import numpy as np
import ml_dtypes


def mxq(x, axis, fmt="e4m3"):
    dtype, down = {"e4m3": (ml_dtypes.float8_e4m3fn, 7), "e5m2": (ml_dtypes.float8_e5m2, 14)}[fmt]
    v = np.moveaxis(np.asarray(x, np.float32).astype(ml_dtypes.bfloat16).astype(np.float64), axis, -1)
    blocks = v.reshape(v.shape[:-1] + (-1, 32))
    amax = np.abs(blocks).max(-1, keepdims=True)
    byte = np.maximum(np.where(amax > 0, np.frexp(amax)[1] - 1 + 127, 0) - down, 1)
    scale = np.exp2(byte - 127.0)
    codes = (blocks / scale).astype(np.float32).astype(dtype).astype(np.float64)
    return np.moveaxis((codes * scale).reshape(v.shape), -1, axis)


WIDE = False


def mx_kscale(k):
    if not WIDE:
        return np.ones(k)
    levels = np.array([10, -10, 5, -5, 0])
    if k % 512:
        return np.exp2(np.random.permutation(np.resize(levels, k // 32))).repeat(32)
    a = np.empty((k // 512, 16))
    for p in range(k // 512):
        a[p, :8] = np.random.permutation(np.resize(levels, 8))
        for g in range(8):
            far = levels[np.abs(levels - a[p, g]) >= 10]
            a[p, g + 8] = far[np.random.randint(len(far))]
    return np.exp2(a.ravel()).repeat(32)


BF16 = ml_dtypes.bfloat16


def bf(x):
    return np.asarray(x, np.float32).astype(BF16)


def f64(x):
    return np.asarray(x).astype(np.float64)


E2M1 = np.array([0.0, 0.5, 1.0, 1.5, 2.0, 3.0, 4.0, 6.0, -0.0, -0.5, -1.0, -1.5, -2.0, -3.0, -4.0, -6.0])


def pack_weight(w, fmt):
    k, n = w.shape
    w = f64(bf(w)).reshape(k // 32, 32, n)
    amax = np.abs(w).max(1)
    if fmt == "e4m3":
        byte = np.frexp(amax)[1] - 1 + 127 - 7
    else:
        mant, ex = np.frexp(amax / 6.0)
        byte = np.where(mant > 0.5, ex, ex - 1) + 127
    byte = np.clip(np.where(amax > 0, byte, 1), 1, 254)
    scaled = (w * np.exp2(127.0 - byte)[:, None, :]).reshape(k, n).astype(np.float32)
    by_word = np.ascontiguousarray(scaled.reshape(k // 512, 128, 4, n).transpose(0, 1, 3, 2))
    if fmt == "e4m3":
        words = by_word.astype(ml_dtypes.float8_e4m3fn).view(np.uint8)
    else:
        c = by_word.astype(ml_dtypes.float4_e2m1fn).view(np.uint8) & 0xF
        words = c[..., 0::2] | (c[..., 1::2] << 4)
    return np.ascontiguousarray(words), np.ascontiguousarray(byte.astype(np.uint8).reshape(k // 512, 16, n))


def unpack_weight(words, scales, fmt):
    g, p, n, _ = words.shape
    if fmt == "e4m3":
        vals = np.ascontiguousarray(words).view(ml_dtypes.float8_e4m3fn).astype(np.float64)
    else:
        nib = np.empty((g, p, n, 4), np.uint8)
        nib[..., 0::2] = words & 0xF
        nib[..., 1::2] = words >> 4
        vals = E2M1[nib]
    vals = vals * np.repeat(np.exp2(scales.astype(np.float64) - 127.0), 8, axis=1)[..., None]
    return vals.transpose(0, 1, 3, 2).reshape(g * 512, n)
def pack4(w):
    words, scales = pack_weight(w, "e2m1")
    return words.reshape(words.shape[0], 128, -1), scales


def unpack4(words, scales):
    return unpack_weight(words.reshape(words.shape[0], 128, -1, 2), scales, "e2m1")


B, X, N, OS = 2048, 512, 2304, 256
H = N - OS


def draw0():
    s, t = mx_kscale(X), mx_kscale(H)
    std0 = np.sqrt(2.0 / X)
    std1 = np.sqrt(2.0 / (X + H))
    row_scale = np.concatenate([std0 * t, np.full(OS, std1)])
    bias_scale = np.concatenate([t, np.ones(OS)])
    x = bf(np.random.standard_normal((B, X)) * s)
    w0_words, w0_scales = pack4((np.random.standard_normal((N, X)) * row_scale[:, None] / s).T)
    w1_words, w1_scales = pack4((np.random.standard_normal((OS, H)) * std1 / t).T)
    return {"x": x,
            "w0_words": w0_words, "w0_scales": w0_scales,
            "w1_words": w1_words, "w1_scales": w1_scales,
            "biases": bf(np.random.random(N) * bias_scale)}


def core(x, w0_words, w0_scales, w1_words, w1_scales, biases):
    n = w0_scales.shape[2]
    os_ = w1_scales.shape[2]
    z = (mxq(f64(x), 1, "e4m3") @ unpack4(w0_words, w0_scales)) + f64(biases)
    h = np.maximum(z[:, : n - os_], 0.0)
    return z[:, n - os_:] + (mxq(h, 1, "e4m3") @ unpack4(w1_words, w1_scales))


def e4m3fn_bytes(y):
    return np.clip(np.asarray(y, np.float64), -448.0, 448.0).astype(np.float32).astype(ml_dtypes.float8_e4m3fn).view(np.uint8)


def e4m3fn_values(b):
    return np.asarray(b, np.uint8).view(ml_dtypes.float8_e4m3fn).astype(np.float64)


def setup_inputs():
    d = draw0()
    x0 = np.asarray(d['x']).astype(np.float64)
    s = (np.max(np.abs(x0), axis=(0,), keepdims=True) / 448.0).astype(np.float32)
    out = {}
    for k, v in d.items():
        if k == 'x':
            out['x_bytes'] = e4m3fn_bytes(x0 / s.astype(np.float64))
            out['x_scale'] = s
        else:
            out[k] = v
    return out


def reference(x_bytes, x_scale, w0_words, w0_scales, w1_words, w1_scales, biases):
    return core(e4m3fn_values(x_bytes) * x_scale.astype(np.float64), w0_words, w0_scales, w1_words, w1_scales, biases)

@@ -1,0 +1,349 @@
+from contextlib import ExitStack
+
+import concourse.mybir as mybir
+from concourse.masks import make_identity
+
+F32 = mybir.dt.float32
+BF16 = mybir.dt.bfloat16
+U32 = mybir.dt.uint32
+I32 = mybir.dt.int32
+U8 = mybir.dt.uint8
+FP8 = mybir.dt.float8_e4m3fn
+FP8X4 = mybir.dt.float8_e4m3fn_x4
+FP4X4 = mybir.dt.float4_e2m1fn_x4
+RELU = mybir.ActivationFunctionType.Relu
+MULT = mybir.AluOpType.mult
+ADD = mybir.AluOpType.add
+
+P = 128
+B, X, N, OS = 2048, 512, 2304, 256
+H = N - OS
+G = H // 512
+FLOPS = 2 * B * X * N + 2 * B * H * OS
+
+CHUNKS = (2, 4, 4, 4, 2)
+UNITS = tuple((c, g) for c in range(5) for g in range(4))
+SHARE = ((48, 32, 32, 32), (0, 0, 0, 0), (0, 0, 0, 0), (0, 0, 0, 0), (0, 32, 64, 96))
+VE = ()
+CE = 0
+VX = ()
+SC = (0, 1)
+HV = (2, 2, 2, 2, 2)
+SP = 1
+OL = (20, 20)
+WARM = (4, 3)
+XM = ((), (0, 0, 0, 0), (2, 2, 3, 3), (6, 6, 7, 7), (10, 10))
+XT = (0, 0, 5, 9, 13)
+XQ = (0, 1, 6, 10, 14)
+S2 = ((6,), (10, 11), (14, 15), (18, 19))
+PERM = (-2, -2, -1, 0)
+
+
+def tile_spn_w4_kernel(tc, x_bytes, x_scale, w0_words, w0_scales, w1_words, w1_scales, biases, out):
+    nc = tc.nc
+    n_chunks = len(CHUNKS)
+    first = [sum(CHUNKS[:c]) for c in range(n_chunks)]
+    x_view = x_bytes.rearrange("(p j) k -> p j k", j=B // P)
+    out_view = out.rearrange("(p j) n -> p j n", j=B // P)
+
+    with ExitStack() as ctx:
+        keep = ctx.enter_context(tc.tile_pool(name="keep", bufs=1))
+        work = ctx.enter_context(tc.tile_pool(name="work", bufs=4))
+        psum = ctx.enter_context(tc.psum_pool(name="psum", bufs=5))
+        ctx.enter_context(tc.manual_schedule())
+
+        ident = keep.tile([P, P], F32, name="ident")
+        xs = keep.tile([P, X], F32, name="xs")
+        w0_raw = keep.tile([P, 2 * N], U8, name="w0_raw", align_bytes=64)
+        w0s_raw = keep.tile([P, N], U8, name="w0s_raw", align_bytes=64)
+        w0_perm = keep.tile([P, 2 * H], U8, name="w0_perm", align_bytes=64)
+        w0s_perm = keep.tile([P, H], U8, name="w0s_perm", align_bytes=64)
+        w1 = keep.tile([P, G, 2 * OS], U8, name="w1", align_bytes=64)
+        w1s = keep.tile([P, G, OS], U8, name="w1s", align_bytes=64)
+        bias_h = keep.tile([P, G, 4], BF16, name="bias_h")
+        bias_o = keep.tile([P, OS], BF16, name="bias_o")
+        xs_col = keep.tile([P, 4], F32, name="xs_col")
+        warm = keep.tile([P, 1], F32, name="warm")
+        xb = []
+        for c in range(n_chunks):
+            xb_c = keep.tile([P, CHUNKS[c], X], U8, name="xbytes%d" % c, align_bytes=64)
+            xb.append(xb_c)
+
+        zeros = keep.tile([P, 512], BF16, name="zeros")
+        nc.vector.memset(zeros[:], 0.0)
+        nc.vector.memset(w0s_raw[:].bitcast(I32), 0)
+        nc.vector.memset(warm[:], 0.0)
+        nc.vector.memset(w1s[:].rearrange("p g n -> p (g n)").bitcast(I32), 0)
+        make_identity(nc, ident[:])
+
+        def load_x(c):
+            nc.sync.dma_start(out=xb[c][:], in_=x_view[:, first[c] : first[c] + CHUNKS[c], :])
+
+        nc.scalar.activation(out=warm[:], in_=warm[:], func=RELU)
+        load_x(0)
+        nc.sync.dma_start(out=xs_col[:], in_=x_scale.rearrange("o (n m) -> n (o m)", m=4))
+        nc.sync.dma_start(out=w0_raw[:, 0:1024], in_=w0_words[0, :, 0:1024])
+        for q in range(4):
+            nc.sync.dma_start(
+                out=w0s_raw[32 * q : 32 * q + 4, :].bitcast(I32),
+                in_=w0_scales[0, 4 * q : 4 * q + 4, :].bitcast(I32),
+            )
+        load_x(1)
+        nc.scalar.dma_start(out=bias_h[:], in_=biases[0:H].rearrange("(g p t) -> p g t", g=G, p=P, t=4))
+        nc.sync.dma_start(out=w0_raw[:, 1024:2048], in_=w0_words[0, :, 1024:2048])
+        nc.sync.dma_start(out=w0_raw[:, 2048:4608], in_=w0_words[0, :, 2048:4608])
+        nc.sync.dma_start(out=w1[:], in_=w1_words.rearrange("g p n -> p g n"))
+        for q in range(4):
+            nc.sync.dma_start(
+                out=w1s[32 * q : 32 * q + 4].bitcast(I32),
+                in_=w1_scales[:, 4 * q : 4 * q + 4, :].rearrange("g r n -> r g n").bitcast(I32),
+            )
+        for c in range(2, n_chunks):
+            load_x(c)
+        nc.sync.dma_start(out=bias_o[:], in_=biases[H:N].partition_broadcast(P))
+
+        xv, xg, xq, xqs = {}, {}, {}, {}
+        xt = {}
+        hp, hg, hq, hqs, acc = {}, {}, {}, {}, {}
+
+        def permute_codes(g):
+            nc.vector.tensor_copy(
+                out=w0_perm[:, 1024 * g : 1024 * (g + 1)].rearrange("p (t m b) -> p t m b", t=4, b=2),
+                in_=w0_raw[:, 1024 * g : 1024 * (g + 1)].rearrange("p (m t b) -> p t m b", t=4, b=2),
+            )
+
+        def permute_scales(engine, g, t0, t1):
+            engine.tensor_copy(
+                out=w0s_perm[:, 512 * g : 512 * (g + 1)].rearrange("p (t m) -> p t m", t=4)[:, t0:t1],
+                in_=w0s_raw[:, 512 * g : 512 * (g + 1)].rearrange("p (m t) -> p t m", t=4)[:, t0:t1],
+            )
+
+        def x_mult(c, j):
+            t = work.tile([P, X], BF16, name="xv", bufs=8, align_bytes=64)
+            xv[c, j] = t
+            nc.vector.tensor_tensor(out=t[:], in0=xb[c][:, j, :].bitcast(FP8), in1=xs[:], op=MULT)
+
+        def x_cast(c, j):
+            t = work.tile([P, X], BF16, name="xv", bufs=8, align_bytes=64)
+            xv[c, j] = t
+            (nc.scalar.copy if c or CE else nc.vector.tensor_copy)(out=t[:], in_=xb[c][:, j, :].bitcast(FP8))
+
+        def x_scale_out(c, j):
+            if j == 0:
+                xg[c] = work.tile([P, 2048], BF16, name="xg", bufs=2, align_bytes=64)
+            nc.vector.tensor_tensor(
+                out=xg[c][:, 512 * j : 512 * (j + 1)].rearrange("p (r u e) -> p r u e", u=2, e=2),
+                in0=xt[c, j // 2][:, j % 2].rearrange("p u r -> p (u r)").bitcast(BF16).rearrange("p (u r e) -> p r u e", u=2, e=2),
+                in1=xs_col[:].rearrange("p (o u e) -> p o u e", o=1, u=2).to_broadcast([P, P, 2, 2]),
+                op=MULT,
+            )
+
+        def x_transpose(c, pair):
+            t = psum.tile([P, 2, 2, P], F32, name="xt", tag="xo", bufs=3)
+            xt[c, pair] = t
+            for jj in range(min(2, CHUNKS[c] - 2 * pair)):
+                words = xv[c, 2 * pair + jj][:].bitcast(F32)
+                for u in range(2):
+                    nc.tensor.transpose(t[:, jj, u, :], words[:, u : X // 2 : 2], ident[:])
+
+        def x_copy(c, pair):
+            if pair == 0:
+                xg[c] = work.tile([P, 2048], BF16, name="xg", bufs=2, align_bytes=64)
+            k = min(2, CHUNKS[c] - 2 * pair)
+            move = nc.vector.tensor_copy if (c, pair) in VX else nc.scalar.copy
+            move(
+                out=xg[c][:, 1024 * pair : 1024 * pair + 512 * k].bitcast(F32).rearrange("p (j r u) -> p j r u", j=k, u=2),
+                in_=xt[c, pair][:, :k].rearrange("p j u r -> p j r u"),
+            )
+
+        def x_quantize(c):
+            n = CHUNKS[c] * P
+            xq[c] = work.tile([P, 512], U32, name="xq", bufs=n_chunks, align_bytes=64)
+            xqs[c] = work.tile([P, 512], U8, name="xqs", bufs=n_chunks, align_bytes=64)
+            nc.vector.quantize_mx(out=xq[c][:, :n].bitcast(FP8X4), scales=xqs[c][:, :n], in_=xg[c][:, : 4 * n])
+
+        def stage1(c, g):
+            n = CHUNKS[c] * P
+            h = work.tile([P, 4, 512], BF16, name="hp", bufs=4, align_bytes=64)
+            hp[c, g] = h
+            for t in range(4):
+                z = psum.tile([P, 512], F32, name="z", bufs=5)
+                m0 = 512 * g + P * t
+                nc.tensor.matmul_mx(
+                    out=z[:, :n],
+                    lhsT=w0_perm[:, 2 * m0 : 2 * (m0 + P)].bitcast(FP4X4),
+                    lhsT_scale=w0s_perm[:, m0 : m0 + P],
+                    rhs=xq[c][:, :n].bitcast(FP8X4),
+                    rhs_scale=xqs[c][:, :n],
+                    start=True,
+                    stop=True,
+                )
+                if t == 3 and (c, g) in VE:
+                    nc.vector.tensor_scalar(out=h[:, t, :n], in0=z[:, :n], scalar1=bias_h[:, g, t : t + 1], scalar2=0.0, op0=ADD, op1=mybir.AluOpType.max)
+                else:
+                    nc.scalar.activation(out=h[:, t, :n], in_=z[:, :n], func=RELU, bias=bias_h[:, g, t : t + 1])
+            hg[c, g] = work.tile([P, 2048], BF16, name="hg", bufs=4, align_bytes=64)
+            weave(nc.scalar.copy, c, g, n - SHARE[c][g], n)
+
+        def weave(engine_copy, c, g, a, b):
+            if b > a:
+                engine_copy(
+                    out=hg[c, g][:, 4 * a : 4 * b].rearrange("p (c i t) -> p c t i", t=4, i=4),
+                    in_=hp[c, g][:, :, a:b].rearrange("p t (c i) -> p c t i", i=4),
+                )
+
+        def h_quantize(c, g, half):
+            n = CHUNKS[c] * P // halves[c]
+            if half == 0:
+                hq[c, g] = work.tile([P, 512], U32, name="hq", bufs=12, align_bytes=64)
+                hqs[c, g] = work.tile([P, 512], U8, name="hqs", bufs=12, align_bytes=64)
+            a = half * n
+            nc.vector.quantize_mx(
+                out=hq[c, g][:, a : a + n].bitcast(FP8X4),
+                scales=hqs[c, g][:, a : a + n],
+                in_=hg[c, g][:, 4 * a : 4 * (a + n)],
+            )
+
+        def pass2(dst, c, j, half, opens, groups, closes):
+            cols = slice(j * P, (j + 1) * P)
+            n0 = H + half * P
+            if opens:
+                nc.tensor.matmul_mx(
+                    out=dst,
+                    lhsT=xq[c][:, cols].bitcast(FP8X4),
+                    lhsT_scale=xqs[c][:, cols],
+                    rhs=w0_raw[:, 2 * n0 : 2 * (n0 + P)].bitcast(FP4X4),
+                    rhs_scale=w0s_raw[:, n0 : n0 + P],
+                    start=True,
+                    stop=False,
+                )
+            for g in groups:
+                nc.tensor.matmul_mx(
+                    out=dst,
+                    lhsT=hq[c, g][:, cols].bitcast(FP8X4),
+                    lhsT_scale=hqs[c, g][:, cols],
+                    rhs=w1[:, g, 2 * half * P : 2 * (half + 1) * P].bitcast(FP4X4),
+                    rhs_scale=w1s[:, g, half * P : (half + 1) * P],
+                    start=False,
+                    stop=(closes and g == groups[-1]),
+                )
+
+        def stage2(c, j0, count):
+            o = psum.tile([P, 2, OS], F32, name="o", tag="xo", bufs=3)
+            acc[c, j0] = o
+            for jj in range(count):
+                for half in range(2):
+                    pass2(o[:, jj, half * P : (half + 1) * P], c, j0 + jj, half, True, range(G), True)
+
+        def finish(c, j0, count):
+            res = work.tile([P, 2, OS], F32, name="res", bufs=4)
+            nc.vector.tensor_tensor(
+                out=res[:, :count, :],
+                in0=acc[c, j0][:, :count, :],
+                in1=bias_o[:].unsqueeze(1).to_broadcast([P, count, OS]),
+                op=ADD,
+            )
+            nc.sync.dma_start(out=out_view[:, first[c] + j0 : first[c] + j0 + count, :], in_=res[:, :count, :])
+
+        last = n_chunks - 1
+        tail = {}
+
+        def open_last(j):
+            for half in range(2):
+                tag, bufs = ("xo", 3) if j == 0 else ("z", 5)
+                o = psum.tile([P, P], F32, name="tail", tag=tag, bufs=bufs)
+                tail[j, half] = o
+                pass2(o[:], last, j, half, True, range(G - 1), False)
+
+        def close_last(j):
+            for half in range(2):
+                pass2(tail[j, half][:], last, j, half, False, (G - 1,), True)
+
+        def finish_last(j):
+            res = work.tile([P, OS], F32, name="tail_res", bufs=2)
+            for half in range(2):
+                cols = slice(half * P, (half + 1) * P)
+                nc.vector.tensor_tensor(out=res[:, cols], in0=tail[j, half][:], in1=bias_o[:, cols], op=ADD)
+            nc.sync.dma_start(out=out_view[:, first[last] + j, :], in_=res[:])
+
+        def spread_scales():
+            spread = psum.tile([P, 4, P], F32, name="spread", tag="xo", bufs=3)
+            for m in range(4):
+                nc.tensor.transpose(spread[:, m, :], xs_col[:, m : m + 1].to_broadcast([P, P]), ident[:])
+            nc.scalar.copy(out=xs[:].rearrange("p (n m) -> p n m", m=4), in_=spread[:].rearrange("p m n -> p n m"))
+
+        def dummies(k):
+            d = psum.tile([P, 512], F32, name="z", bufs=5)
+            for i in range(k):
+                nc.tensor.matmul(d[:], lhsT=zeros[:, :P], rhs=zeros[:], start=True, stop=True)
+
+        n_units = len(UNITS)
+        vec, mid, ten = {}, {}, {}
+
+        def put(table, s, f, *args):
+            table.setdefault(s, []).append((f, args))
+
+        def run(table, s):
+            for f, args in table.get(s, []):
+                f(*args)
+
+        halves = [HV[c] for c in range(n_chunks)]
+        pairs = [(r + 1) // 2 for r in CHUNKS]
+        for g in range(1, G):
+            put(vec, PERM[g], permute_codes, g)
+            put(vec, PERM[g], permute_scales, nc.vector, g, 0, 4)
+        for c in range(1, n_chunks):
+            for j in range(CHUNKS[c]):
+                put(vec, XM[c][j], x_scale_out if c in SC else x_mult, c, j)
+            for pair in range(pairs[c]):
+                if c not in SC:
+                    put(ten, XT[c], x_transpose, c, pair)
+                    put(ten, XT[c], x_copy, c, pair)
+            put(mid, XQ[c], x_quantize, c)
+        for c in range(last):
+            for i in range(pairs[c]):
+                k = min(2, CHUNKS[c] - 2 * i)
+                put(ten, S2[c][i], stage2, c, 2 * i, k)
+                put(vec if c == last - 1 else mid, S2[c][i] + 1, finish, c, 2 * i, k)
+        for j in range(CHUNKS[last]):
+            put(ten, OL[j], open_last, j)
+        put(ten, SP, spread_scales)
+
+        dummies(WARM[0])
+        for c in SC:
+            for j in range(CHUNKS[c]):
+                x_cast(c, j)
+        x_transpose(0, 0)
+        for c in SC[1:]:
+            for pair in range(pairs[c]):
+                put(ten, XT[c], x_transpose, c, pair)
+        if WARM[1]:
+            dummies(WARM[1])
+        permute_codes(0)
+        for j in range(CHUNKS[0]):
+            x_scale_out(0, j)
+        permute_scales(nc.vector, 0, 0, 4)
+        x_quantize(0)
+        run(vec, -2)
+        run(vec, -1)
+
+        for s in range(n_units + 1):
+            if s < n_units:
+                stage1(*UNITS[s])
+            if s > 0:
+                c, g = UNITS[s - 1]
+                n = CHUNKS[c] * P
+                cut = n // halves[c]
+                end = n - SHARE[c][g]
+                weave(nc.vector.tensor_copy, c, g, 0, min(cut, end))
+                weave(nc.vector.tensor_copy, c, g, cut, end)
+            run(mid, s)
+            if s > 0:
+                h_quantize(c, g, 0)
+                if halves[c] == 2:
+                    h_quantize(c, g, 1)
+            run(ten, s)
+            run(vec, s)
+        for j in range(CHUNKS[last]):
+            close_last(j)
+            finish_last(j)

@@ -22,27 +22,21 @@ G = H // 512
 FLOPS = 2 * B * X * N + 2 * B * H * OS
 
 CHUNKS = (2, 4, 4, 4, 2)
-UNITS = tuple((c, g) for c in range(5) for g in range(4))
-SHARE = ((48, 32, 32, 32), (0, 0, 0, 0), (0, 0, 0, 0), (0, 0, 0, 0), (0, 32, 64, 96))
-VE = ()
-CE = 0
-VX = ()
-SC = (0, 1)
-HV = (2, 2, 2, 2, 2)
-SP = 1
-OL = (20, 20)
+HEAD_CHUNKS = 2
+SHARE_MID = (0,0,0,0)
+SHARE_HEAD = (0,0,0,0)
+SHARE_TAIL = (0,0,64,128)
 WARM = (4, 3)
-XM = ((), (0, 0, 0, 0), (2, 2, 3, 3), (6, 6, 7, 7), (10, 10))
-XT = (0, 0, 5, 9, 13)
-XQ = (0, 1, 6, 10, 14)
-S2 = ((6,), (10, 11), (14, 15), (18, 19))
-PERM = (-2, -2, -1, 0)
+HEAD_V_CASTS = 2
 
 
 def tile_spn_w4_kernel(tc, x_bytes, x_scale, w0_words, w0_scales, w1_words, w1_scales, biases, out):
     nc = tc.nc
     n_chunks = len(CHUNKS)
+    last = n_chunks - 1
     first = [sum(CHUNKS[:c]) for c in range(n_chunks)]
+    units = [(c, g) for c in range(n_chunks) for g in range(G)]
+    n_units = len(units)
     x_view = x_bytes.rearrange("(p j) k -> p j k", j=B // P)
     out_view = out.rearrange("(p j) n -> p j n", j=B // P)
 
@@ -63,47 +57,51 @@ def tile_spn_w4_kernel(tc, x_bytes, x_scale, w0_words, w0_scales, w1_words, w1_s
         bias_h = keep.tile([P, G, 4], BF16, name="bias_h")
         bias_o = keep.tile([P, OS], BF16, name="bias_o")
         xs_col = keep.tile([P, 4], F32, name="xs_col")
-        warm = keep.tile([P, 1], F32, name="warm")
         xb = []
         for c in range(n_chunks):
             xb_c = keep.tile([P, CHUNKS[c], X], U8, name="xbytes%d" % c, align_bytes=64)
             xb.append(xb_c)
 
-        zeros = keep.tile([P, 512], BF16, name="zeros")
-        nc.vector.memset(zeros[:], 0.0)
+        if WARM:
+            zeros = keep.tile([P, 512], BF16, name="zeros")
+            warm = keep.tile([P, 1], F32, name="warm")
+            nc.vector.memset(zeros[:], 0.0)
         nc.vector.memset(w0s_raw[:].bitcast(I32), 0)
-        nc.vector.memset(warm[:], 0.0)
+        if WARM:
+            nc.vector.memset(warm[:], 0.0)
         nc.vector.memset(w1s[:].rearrange("p g n -> p (g n)").bitcast(I32), 0)
         make_identity(nc, ident[:])
 
         def load_x(c):
             nc.sync.dma_start(out=xb[c][:], in_=x_view[:, first[c] : first[c] + CHUNKS[c], :])
 
-        nc.scalar.activation(out=warm[:], in_=warm[:], func=RELU)
+        if WARM:
+            nc.scalar.activation(out=warm[:], in_=warm[:], func=RELU)
         load_x(0)
-        nc.sync.dma_start(out=xs_col[:], in_=x_scale.rearrange("o (n m) -> n (o m)", m=4))
         nc.sync.dma_start(out=w0_raw[:, 0:1024], in_=w0_words[0, :, 0:1024])
+        nc.sync.dma_start(out=xs_col[:], in_=x_scale.rearrange("o (n m) -> n (o m)", m=4))
+        pass
         for q in range(4):
             nc.sync.dma_start(
                 out=w0s_raw[32 * q : 32 * q + 4, :].bitcast(I32),
                 in_=w0_scales[0, 4 * q : 4 * q + 4, :].bitcast(I32),
             )
         load_x(1)
-        nc.scalar.dma_start(out=bias_h[:], in_=biases[0:H].rearrange("(g p t) -> p g t", g=G, p=P, t=4))
+        nc.sync.dma_start(out=bias_h[:], in_=biases[0:H].rearrange("(g p t) -> p g t", g=G, p=P, t=4))
         nc.sync.dma_start(out=w0_raw[:, 1024:2048], in_=w0_words[0, :, 1024:2048])
         nc.sync.dma_start(out=w0_raw[:, 2048:4608], in_=w0_words[0, :, 2048:4608])
+        load_x(2)
         nc.sync.dma_start(out=w1[:], in_=w1_words.rearrange("g p n -> p g n"))
         for q in range(4):
             nc.sync.dma_start(
                 out=w1s[32 * q : 32 * q + 4].bitcast(I32),
                 in_=w1_scales[:, 4 * q : 4 * q + 4, :].rearrange("g r n -> r g n").bitcast(I32),
             )
-        for c in range(2, n_chunks):
+        for c in range(3, n_chunks):
             load_x(c)
         nc.sync.dma_start(out=bias_o[:], in_=biases[H:N].partition_broadcast(P))
 
-        xv, xg, xq, xqs = {}, {}, {}, {}
-        xt = {}
+        xv, xt, xg, xq, xqs = {}, {}, {}, {}, {}
         hp, hg, hq, hqs, acc = {}, {}, {}, {}, {}
 
         def permute_codes(g):
@@ -112,10 +110,10 @@ def tile_spn_w4_kernel(tc, x_bytes, x_scale, w0_words, w0_scales, w1_words, w1_s
                 in_=w0_raw[:, 1024 * g : 1024 * (g + 1)].rearrange("p (m t b) -> p t m b", t=4, b=2),
             )
 
-        def permute_scales(engine, g, t0, t1):
-            engine.tensor_copy(
-                out=w0s_perm[:, 512 * g : 512 * (g + 1)].rearrange("p (t m) -> p t m", t=4)[:, t0:t1],
-                in_=w0s_raw[:, 512 * g : 512 * (g + 1)].rearrange("p (m t) -> p t m", t=4)[:, t0:t1],
+        def permute_scales(g):
+            nc.vector.tensor_copy(
+                out=w0s_perm[:, 512 * g : 512 * (g + 1)].rearrange("p (t m) -> p t m", t=4),
+                in_=w0s_raw[:, 512 * g : 512 * (g + 1)].rearrange("p (m t) -> p t m", t=4),
             )
 
         def x_mult(c, j):
@@ -123,10 +121,18 @@ def tile_spn_w4_kernel(tc, x_bytes, x_scale, w0_words, w0_scales, w1_words, w1_s
             xv[c, j] = t
             nc.vector.tensor_tensor(out=t[:], in0=xb[c][:, j, :].bitcast(FP8), in1=xs[:], op=MULT)
 
-        def x_cast(c, j):
+        def x_cast(c, j, move):
             t = work.tile([P, X], BF16, name="xv", bufs=8, align_bytes=64)
             xv[c, j] = t
-            (nc.scalar.copy if c or CE else nc.vector.tensor_copy)(out=t[:], in_=xb[c][:, j, :].bitcast(FP8))
+            move(out=t[:], in_=xb[c][:, j, :].bitcast(FP8))
+
+        def x_transpose(c, pair):
+            t = psum.tile([P, 2, 2, P], F32, name="xt", tag="xo", bufs=3)
+            xt[c, pair] = t
+            for jj in range(2):
+                words = xv[c, 2 * pair + jj][:].bitcast(F32)
+                for u in range(2):
+                    nc.tensor.transpose(t[:, jj, u, :], words[:, u : X // 2 : 2], ident[:])
 
         def x_scale_out(c, j):
             if j == 0:
@@ -138,22 +144,12 @@ def tile_spn_w4_kernel(tc, x_bytes, x_scale, w0_words, w0_scales, w1_words, w1_s
                 op=MULT,
             )
 
-        def x_transpose(c, pair):
-            t = psum.tile([P, 2, 2, P], F32, name="xt", tag="xo", bufs=3)
-            xt[c, pair] = t
-            for jj in range(min(2, CHUNKS[c] - 2 * pair)):
-                words = xv[c, 2 * pair + jj][:].bitcast(F32)
-                for u in range(2):
-                    nc.tensor.transpose(t[:, jj, u, :], words[:, u : X // 2 : 2], ident[:])
-
         def x_copy(c, pair):
             if pair == 0:
                 xg[c] = work.tile([P, 2048], BF16, name="xg", bufs=2, align_bytes=64)
-            k = min(2, CHUNKS[c] - 2 * pair)
-            move = nc.vector.tensor_copy if (c, pair) in VX else nc.scalar.copy
-            move(
-                out=xg[c][:, 1024 * pair : 1024 * pair + 512 * k].bitcast(F32).rearrange("p (j r u) -> p j r u", j=k, u=2),
-                in_=xt[c, pair][:, :k].rearrange("p j u r -> p j r u"),
+            nc.scalar.copy(
+                out=xg[c][:, 1024 * pair : 1024 * (pair + 1)].bitcast(F32).rearrange("p (j r u) -> p j r u", j=2, u=2),
+                in_=xt[c, pair][:].rearrange("p j u r -> p j r u"),
             )
 
         def x_quantize(c):
@@ -162,108 +158,75 @@ def tile_spn_w4_kernel(tc, x_bytes, x_scale, w0_words, w0_scales, w1_words, w1_s
             xqs[c] = work.tile([P, 512], U8, name="xqs", bufs=n_chunks, align_bytes=64)
             nc.vector.quantize_mx(out=xq[c][:, :n].bitcast(FP8X4), scales=xqs[c][:, :n], in_=xg[c][:, : 4 * n])
 
-        def stage1(c, g):
+        def share(s):
+            c, g = units[s]
+            return SHARE_HEAD[g] if c == 0 else SHARE_TAIL[g] if c == last else SHARE_MID[g] if c < 3 else 0
+
+        def plane(s, t):
+            c, g = units[s]
             n = CHUNKS[c] * P
-            h = work.tile([P, 4, 512], BF16, name="hp", bufs=4, align_bytes=64)
-            hp[c, g] = h
-            for t in range(4):
-                z = psum.tile([P, 512], F32, name="z", bufs=5)
-                m0 = 512 * g + P * t
-                nc.tensor.matmul_mx(
-                    out=z[:, :n],
-                    lhsT=w0_perm[:, 2 * m0 : 2 * (m0 + P)].bitcast(FP4X4),
-                    lhsT_scale=w0s_perm[:, m0 : m0 + P],
-                    rhs=xq[c][:, :n].bitcast(FP8X4),
-                    rhs_scale=xqs[c][:, :n],
-                    start=True,
-                    stop=True,
-                )
-                if t == 3 and (c, g) in VE:
-                    nc.vector.tensor_scalar(out=h[:, t, :n], in0=z[:, :n], scalar1=bias_h[:, g, t : t + 1], scalar2=0.0, op0=ADD, op1=mybir.AluOpType.max)
-                else:
-                    nc.scalar.activation(out=h[:, t, :n], in_=z[:, :n], func=RELU, bias=bias_h[:, g, t : t + 1])
-            hg[c, g] = work.tile([P, 2048], BF16, name="hg", bufs=4, align_bytes=64)
-            weave(nc.scalar.copy, c, g, n - SHARE[c][g], n)
+            if t == 0:
+                hp[s] = work.tile([P, 4, 512], BF16, name="hp", bufs=6, align_bytes=64)
+                hg[s] = work.tile([P, 2048], BF16, name="hg", bufs=6, align_bytes=64)
+            z = psum.tile([P, 512], F32, name="z", bufs=5)
+            m0 = 512 * g + P * t
+            nc.tensor.matmul_mx(
+                out=z[:, :n],
+                lhsT=w0_perm[:, 2 * m0 : 2 * (m0 + P)].bitcast(FP4X4),
+                lhsT_scale=w0s_perm[:, m0 : m0 + P],
+                rhs=xq[c][:, :n].bitcast(FP8X4),
+                rhs_scale=xqs[c][:, :n],
+                start=True,
+                stop=True,
+            )
+            nc.scalar.activation(out=hp[s][:, t, :n], in_=z[:, :n], func=RELU, bias=bias_h[:, g, t : t + 1])
 
-        def weave(engine_copy, c, g, a, b):
+        def weave(move, s, a, b):
             if b > a:
-                engine_copy(
-                    out=hg[c, g][:, 4 * a : 4 * b].rearrange("p (c i t) -> p c t i", t=4, i=4),
-                    in_=hp[c, g][:, :, a:b].rearrange("p t (c i) -> p c t i", i=4),
+                move(
+                    out=hg[s][:, 4 * a : 4 * b].rearrange("p (c i t) -> p c t i", t=4, i=4),
+                    in_=hp[s][:, :, a:b].rearrange("p t (c i) -> p c t i", i=4),
                 )
 
-        def h_quantize(c, g, half):
-            n = CHUNKS[c] * P // halves[c]
-            if half == 0:
-                hq[c, g] = work.tile([P, 512], U32, name="hq", bufs=12, align_bytes=64)
-                hqs[c, g] = work.tile([P, 512], U8, name="hqs", bufs=12, align_bytes=64)
-            a = half * n
-            nc.vector.quantize_mx(
-                out=hq[c, g][:, a : a + n].bitcast(FP8X4),
-                scales=hqs[c, g][:, a : a + n],
-                in_=hg[c, g][:, 4 * a : 4 * (a + n)],
-            )
+        def h_quantize(s, a, b):
+            if a == 0:
+                hq[s] = work.tile([P, 512], U32, name="hq", bufs=12, align_bytes=64)
+                hqs[s] = work.tile([P, 512], U8, name="hqs", bufs=12, align_bytes=64)
+            nc.vector.quantize_mx(out=hq[s][:, a:b].bitcast(FP8X4), scales=hqs[s][:, a:b], in_=hg[s][:, 4 * a : 4 * b])
 
-        def pass2(dst, c, j, half, opens, groups, closes):
+        def out_pass(dst, lhs, lhs_scales, j, rhs, rhs_scales, start, stop):
             cols = slice(j * P, (j + 1) * P)
-            n0 = H + half * P
-            if opens:
-                nc.tensor.matmul_mx(
-                    out=dst,
-                    lhsT=xq[c][:, cols].bitcast(FP8X4),
-                    lhsT_scale=xqs[c][:, cols],
-                    rhs=w0_raw[:, 2 * n0 : 2 * (n0 + P)].bitcast(FP4X4),
-                    rhs_scale=w0s_raw[:, n0 : n0 + P],
-                    start=True,
-                    stop=False,
-                )
-            for g in groups:
-                nc.tensor.matmul_mx(
-                    out=dst,
-                    lhsT=hq[c, g][:, cols].bitcast(FP8X4),
-                    lhsT_scale=hqs[c, g][:, cols],
-                    rhs=w1[:, g, 2 * half * P : 2 * (half + 1) * P].bitcast(FP4X4),
-                    rhs_scale=w1s[:, g, half * P : (half + 1) * P],
-                    start=False,
-                    stop=(closes and g == groups[-1]),
-                )
-
-        def stage2(c, j0, count):
-            o = psum.tile([P, 2, OS], F32, name="o", tag="xo", bufs=3)
-            acc[c, j0] = o
-            for jj in range(count):
-                for half in range(2):
-                    pass2(o[:, jj, half * P : (half + 1) * P], c, j0 + jj, half, True, range(G), True)
-
-        def finish(c, j0, count):
-            res = work.tile([P, 2, OS], F32, name="res", bufs=4)
-            nc.vector.tensor_tensor(
-                out=res[:, :count, :],
-                in0=acc[c, j0][:, :count, :],
-                in1=bias_o[:].unsqueeze(1).to_broadcast([P, count, OS]),
-                op=ADD,
+            nc.tensor.matmul_mx(
+                out=dst,
+                lhsT=lhs[:, cols].bitcast(FP8X4),
+                lhsT_scale=lhs_scales[:, cols],
+                rhs=rhs.bitcast(FP4X4),
+                rhs_scale=rhs_scales,
+                start=start,
+                stop=stop,
             )
-            nc.sync.dma_start(out=out_view[:, first[c] + j0 : first[c] + j0 + count, :], in_=res[:, :count, :])
 
-        last = n_chunks - 1
-        tail = {}
+        def stage2(s, tiles):
+            c, g = units[s]
+            per_bank = 1 if c == last else 2
+            for j in tiles:
+                if g == 0:
+                    if j % per_bank == 0:
+                        tag, bufs = ("xo", 3) if c < last or j == 0 else ("z", 5)
+                        acc[c, j // per_bank] = psum.tile([P, per_bank, OS], F32, name="o", tag=tag, bufs=bufs)
+                    out_pass(acc[c, j // per_bank][:, j % per_bank, :], xq[c], xqs[c], j, w0_raw[:, 2 * H : 2 * N], w0s_raw[:, H:N], j % per_bank == 0, False)
+                closes = g == G - 1 and j % per_bank == per_bank - 1
+                out_pass(acc[c, j // per_bank][:, j % per_bank, :], hq[s], hqs[s], j, w1[:, g, :], w1s[:, g, :], False, closes)
 
-        def open_last(j):
-            for half in range(2):
-                tag, bufs = ("xo", 3) if j == 0 else ("z", 5)
-                o = psum.tile([P, P], F32, name="tail", tag=tag, bufs=bufs)
-                tail[j, half] = o
-                pass2(o[:], last, j, half, True, range(G - 1), False)
-
-        def close_last(j):
-            for half in range(2):
-                pass2(tail[j, half][:], last, j, half, False, (G - 1,), True)
+        def finish(c, pair):
+            res = work.tile([P, 2, OS], F32, name="res", bufs=4)
+            nc.vector.tensor_tensor(out=res[:], in0=acc[c, pair][:], in1=bias_o[:].unsqueeze(1).to_broadcast([P, 2, OS]), op=ADD)
+            j0 = first[c] + 2 * pair
+            nc.sync.dma_start(out=out_view[:, j0 : j0 + 2, :], in_=res[:])
 
         def finish_last(j):
             res = work.tile([P, OS], F32, name="tail_res", bufs=2)
-            for half in range(2):
-                cols = slice(half * P, (half + 1) * P)
-                nc.vector.tensor_tensor(out=res[:, cols], in0=tail[j, half][:], in1=bias_o[:, cols], op=ADD)
+            nc.vector.tensor_tensor(out=res[:], in0=acc[last, j][:, 0, :], in1=bias_o[:], op=ADD)
             nc.sync.dma_start(out=out_view[:, first[last] + j, :], in_=res[:])
 
         def spread_scales():
@@ -277,73 +240,103 @@ def tile_spn_w4_kernel(tc, x_bytes, x_scale, w0_words, w0_scales, w1_words, w1_s
             for i in range(k):
                 nc.tensor.matmul(d[:], lhsT=zeros[:, :P], rhs=zeros[:], start=True, stop=True)
 
-        n_units = len(UNITS)
-        vec, mid, ten = {}, {}, {}
-
-        def put(table, s, f, *args):
-            table.setdefault(s, []).append((f, args))
-
-        def run(table, s):
-            for f, args in table.get(s, []):
-                f(*args)
-
-        halves = [HV[c] for c in range(n_chunks)]
-        pairs = [(r + 1) // 2 for r in CHUNKS]
-        for g in range(1, G):
-            put(vec, PERM[g], permute_codes, g)
-            put(vec, PERM[g], permute_scales, nc.vector, g, 0, 4)
-        for c in range(1, n_chunks):
-            for j in range(CHUNKS[c]):
-                put(vec, XM[c][j], x_scale_out if c in SC else x_mult, c, j)
-            for pair in range(pairs[c]):
-                if c not in SC:
-                    put(ten, XT[c], x_transpose, c, pair)
-                    put(ten, XT[c], x_copy, c, pair)
-            put(mid, XQ[c], x_quantize, c)
-        for c in range(last):
-            for i in range(pairs[c]):
-                k = min(2, CHUNKS[c] - 2 * i)
-                put(ten, S2[c][i], stage2, c, 2 * i, k)
-                put(vec if c == last - 1 else mid, S2[c][i] + 1, finish, c, 2 * i, k)
-        for j in range(CHUNKS[last]):
-            put(ten, OL[j], open_last, j)
-        put(ten, SP, spread_scales)
-
-        dummies(WARM[0])
-        for c in SC:
-            for j in range(CHUNKS[c]):
-                x_cast(c, j)
-        x_transpose(0, 0)
-        for c in SC[1:]:
-            for pair in range(pairs[c]):
-                put(ten, XT[c], x_transpose, c, pair)
-        if WARM[1]:
-            dummies(WARM[1])
+        if WARM:
+            dummies(WARM[0])
+        for j in range(CHUNKS[0]):
+            x_cast(0, j, nc.vector.tensor_copy if j >= CHUNKS[0] - HEAD_V_CASTS else nc.scalar.copy)
         permute_codes(0)
+        pass
+        x_transpose(0, 0)
+        spread_scales()
+        if WARM:
+            dummies(WARM[1])
+        for j in range(CHUNKS[1]):
+            x_cast(1, j, nc.scalar.copy)
+        permute_scales(0)
         for j in range(CHUNKS[0]):
             x_scale_out(0, j)
-        permute_scales(nc.vector, 0, 0, 4)
+        pass
         x_quantize(0)
-        run(vec, -2)
-        run(vec, -1)
+        permute_codes(1)
+        permute_scales(1)
+
+        waiting = []
+
+        def vector_step(s, between):
+            n = CHUNKS[units[s][0]] * P
+            end = n - share(s)
+            cuts = (0, n // 2, n) if s == n_units - 1 or (not between and not waiting and s >= 15) else (0, n)
+            for a, b in zip(cuts, cuts[1:]):
+                weave(nc.vector.tensor_copy, s, a, min(b, end))
+            if waiting:
+                between = [(h_quantize, waiting.pop())] + between
+            elif not between and len(cuts) == 2:
+                waiting.append((s, 0, n))
+                return
+            for f, args in between:
+                f(*args)
+            for a, b in zip(cuts, cuts[1:]):
+                h_quantize(s, a, b)
+
+        widths = [CHUNKS[c] * P for c, g in units for t in range(4)]
+
+        def pass_plane(u):
+            c = units[u][0]
+            u = max(u, G * c + (G - 1 if c < last - 1 else 1 if c < last else 0))
+            k = 4 * (u + 1)
+            ahead = 0
+            while k < len(widths) and ahead < (3072 if c < last - 2 else 2048 if c < last - 1 else 1536):
+                ahead = ahead + widths[k]
+                k = k + 1
+            return min(k + 5 - 1, len(widths) - 1)
 
         for s in range(n_units + 1):
-            if s < n_units:
-                stage1(*UNITS[s])
-            if s > 0:
-                c, g = UNITS[s - 1]
-                n = CHUNKS[c] * P
-                cut = n // halves[c]
-                end = n - SHARE[c][g]
-                weave(nc.vector.tensor_copy, c, g, 0, min(cut, end))
-                weave(nc.vector.tensor_copy, c, g, cut, end)
-            run(mid, s)
-            if s > 0:
-                h_quantize(c, g, 0)
-                if halves[c] == 2:
-                    h_quantize(c, g, 1)
-            run(ten, s)
-            run(vec, s)
+            c, g = units[s] if s < n_units else (n_chunks, 0)
+            turn = HEAD_CHUNKS <= c + 1 < n_chunks and g == 1
+            for t in range(4 if s < n_units else 1):
+                if s < n_units:
+                    plane(s, t)
+                if t == 0:
+                    if s > 0:
+                        n1 = CHUNKS[units[s - 1][0]] * P
+                        weave(nc.scalar.copy, s - 1, n1 - share(s - 1), n1)
+                    if s == 1:
+                        for pair in range(CHUNKS[1] // 2):
+                            x_transpose(1, pair)
+                if s < n_units:
+                    for pair in range(2):
+                        for u in range(s - 1):
+                            cu = units[u][0]
+                            if 2 * pair < CHUNKS[cu] and pass_plane(u) + (4 * pair if cu < last - 1 else 0) == 4 * s + t:
+                                stage2(u, (2 * pair, 2 * pair + 1))
+            if turn:
+                for pair in range(CHUNKS[c + 1] // 2):
+                    x_transpose(c + 1, pair)
+                    x_copy(c + 1, pair)
+            if s == 0:
+                for gg in range(2, G):
+                    permute_codes(gg)
+                    permute_scales(gg)
+                continue
+            between = []
+            if s == 1:
+                for j in range(CHUNKS[1]):
+                    x_scale_out(1, j)
+            if s == 1:
+                between.append((x_quantize, (1,)))
+            if g == 2 and HEAD_CHUNKS <= c + 1 < n_chunks:
+                between.append((x_quantize, (c + 1,)))
+            for cf in range(last):
+                pair = s - pass_plane(G * cf + G - 1) // 4 - (1 if cf < last - 1 else 0)
+                if 0 <= pair < CHUNKS[cf] // 2:
+                    between.append((finish, (cf, pair)))
+            cm, gm = divmod(s - 2, G)
+            if HEAD_CHUNKS <= cm + 2 < n_chunks:
+                for j in range(2 * gm, min(2 * gm + 2, CHUNKS[cm + 2])):
+                    between.append((x_mult, (cm + 2, j)))
+            vector_step(s - 1, between)
+            if s == n_units - 1:
+                stage2(s - 1, range(CHUNKS[last]))
         for j in range(CHUNKS[last]):
-            close_last(j)
+            stage2(n_units - 1, (j,))
             finish_last(j)

@@ -106,8 +106,8 @@ def tile_spn_w4_kernel(tc, x_bytes, x_scale, w0_words, w0_scales, w1_words, w1_s
 
         def permute_codes(g):
             nc.vector.tensor_copy(
-                out=w0_perm[:, 1024 * g : 1024 * (g + 1)].rearrange("p (t m b) -> p t m b", t=4, b=2),
-                in_=w0_raw[:, 1024 * g : 1024 * (g + 1)].rearrange("p (m t b) -> p t m b", t=4, b=2),
+                out=w0_perm[:, 1024 * g : 1024 * (g + 1)].bitcast(mybir.dt.uint16).rearrange("p (t m) -> p t m", t=4),
+                in_=w0_raw[:, 1024 * g : 1024 * (g + 1)].bitcast(mybir.dt.uint16).rearrange("p (m t) -> p t m", t=4),
             )
 
         def permute_scales(g):

@@ -7,6 +7,7 @@ F32 = mybir.dt.float32
 BF16 = mybir.dt.bfloat16
 U32 = mybir.dt.uint32
 I32 = mybir.dt.int32
+U16 = mybir.dt.uint16
 U8 = mybir.dt.uint8
 FP8 = mybir.dt.float8_e4m3fn
 FP8X4 = mybir.dt.float8_e4m3fn_x4
@@ -26,8 +27,8 @@ HEAD_CHUNKS = 2
 SHARE_MID = (0,0,0,0)
 SHARE_HEAD = (0,0,0,0)
 SHARE_TAIL = (0,0,64,128)
-WARM = (4, 3)
-HEAD_V_CASTS = 2
+WARM = (5,1,0)
+HEAD_V_CASTS = 1
 
 
 def tile_spn_w4_kernel(tc, x_bytes, x_scale, w0_words, w0_scales, w1_words, w1_scales, biases, out):
@@ -80,13 +81,13 @@ def tile_spn_w4_kernel(tc, x_bytes, x_scale, w0_words, w0_scales, w1_words, w1_s
         load_x(0)
         nc.sync.dma_start(out=w0_raw[:, 0:1024], in_=w0_words[0, :, 0:1024])
         nc.sync.dma_start(out=xs_col[:], in_=x_scale.rearrange("o (n m) -> n (o m)", m=4))
-        pass
+        load_x(1)
         for q in range(4):
             nc.sync.dma_start(
                 out=w0s_raw[32 * q : 32 * q + 4, :].bitcast(I32),
                 in_=w0_scales[0, 4 * q : 4 * q + 4, :].bitcast(I32),
             )
-        load_x(1)
+        pass
         nc.sync.dma_start(out=bias_h[:], in_=biases[0:H].rearrange("(g p t) -> p g t", g=G, p=P, t=4))
         nc.sync.dma_start(out=w0_raw[:, 1024:2048], in_=w0_words[0, :, 1024:2048])
         nc.sync.dma_start(out=w0_raw[:, 2048:4608], in_=w0_words[0, :, 2048:4608])
@@ -106,8 +107,8 @@ def tile_spn_w4_kernel(tc, x_bytes, x_scale, w0_words, w0_scales, w1_words, w1_s
 
         def permute_codes(g):
             nc.vector.tensor_copy(
-                out=w0_perm[:, 1024 * g : 1024 * (g + 1)].bitcast(mybir.dt.uint16).rearrange("p (t m) -> p t m", t=4),
-                in_=w0_raw[:, 1024 * g : 1024 * (g + 1)].bitcast(mybir.dt.uint16).rearrange("p (m t) -> p t m", t=4),
+                out=w0_perm[:, 1024 * g : 1024 * (g + 1)].bitcast(U16).rearrange("p (t m) -> p t m", t=4),
+                in_=w0_raw[:, 1024 * g : 1024 * (g + 1)].bitcast(U16).rearrange("p (m t) -> p t m", t=4),
             )
 
         def permute_scales(g):
@@ -126,11 +127,11 @@ def tile_spn_w4_kernel(tc, x_bytes, x_scale, w0_words, w0_scales, w1_words, w1_s
             xv[c, j] = t
             move(out=t[:], in_=xb[c][:, j, :].bitcast(FP8))
 
-        def x_transpose(c, pair):
-            t = psum.tile([P, 2, 2, P], F32, name="xt", tag="xo", bufs=3)
-            xt[c, pair] = t
-            for jj in range(2):
-                words = xv[c, 2 * pair + jj][:].bitcast(F32)
+        def x_transpose(c, j0, count=2):
+            t = psum.tile([P, count, 2, P], F32, name="xt", tag="xo", bufs=3)
+            for jj in range(count):
+                xt[c, j0 + jj] = (t, jj)
+                words = xv[c, j0 + jj][:].bitcast(F32)
                 for u in range(2):
                     nc.tensor.transpose(t[:, jj, u, :], words[:, u : X // 2 : 2], ident[:])
 
@@ -139,7 +140,7 @@ def tile_spn_w4_kernel(tc, x_bytes, x_scale, w0_words, w0_scales, w1_words, w1_s
                 xg[c] = work.tile([P, 2048], BF16, name="xg", bufs=2, align_bytes=64)
             nc.vector.tensor_tensor(
                 out=xg[c][:, 512 * j : 512 * (j + 1)].rearrange("p (r u e) -> p r u e", u=2, e=2),
-                in0=xt[c, j // 2][:, j % 2].rearrange("p u r -> p (u r)").bitcast(BF16).rearrange("p (u r e) -> p r u e", u=2, e=2),
+                in0=xt[c, j][0][:, xt[c, j][1]].rearrange("p u r -> p (u r)").bitcast(BF16).rearrange("p (u r e) -> p r u e", u=2, e=2),
                 in1=xs_col[:].rearrange("p (o u e) -> p o u e", o=1, u=2).to_broadcast([P, P, 2, 2]),
                 op=MULT,
             )
@@ -149,7 +150,7 @@ def tile_spn_w4_kernel(tc, x_bytes, x_scale, w0_words, w0_scales, w1_words, w1_s
                 xg[c] = work.tile([P, 2048], BF16, name="xg", bufs=2, align_bytes=64)
             nc.scalar.copy(
                 out=xg[c][:, 1024 * pair : 1024 * (pair + 1)].bitcast(F32).rearrange("p (j r u) -> p j r u", j=2, u=2),
-                in_=xt[c, pair][:].rearrange("p j u r -> p j r u"),
+                in_=xt[c, 2 * pair][0][:].rearrange("p j u r -> p j r u"),
             )
 
         def x_quantize(c):
@@ -162,10 +163,10 @@ def tile_spn_w4_kernel(tc, x_bytes, x_scale, w0_words, w0_scales, w1_words, w1_s
             c, g = units[s]
             return SHARE_HEAD[g] if c == 0 else SHARE_TAIL[g] if c == last else SHARE_MID[g] if c < 3 else 0
 
-        def plane(s, t):
+        def plane(s, t, a=0, n=None):
             c, g = units[s]
-            n = CHUNKS[c] * P
-            if t == 0:
+            n = n or CHUNKS[c] * P
+            if t == 0 and a == 0:
                 hp[s] = work.tile([P, 4, 512], BF16, name="hp", bufs=6, align_bytes=64)
                 hg[s] = work.tile([P, 2048], BF16, name="hg", bufs=6, align_bytes=64)
             z = psum.tile([P, 512], F32, name="z", bufs=5)
@@ -174,12 +175,12 @@ def tile_spn_w4_kernel(tc, x_bytes, x_scale, w0_words, w0_scales, w1_words, w1_s
                 out=z[:, :n],
                 lhsT=w0_perm[:, 2 * m0 : 2 * (m0 + P)].bitcast(FP4X4),
                 lhsT_scale=w0s_perm[:, m0 : m0 + P],
-                rhs=xq[c][:, :n].bitcast(FP8X4),
-                rhs_scale=xqs[c][:, :n],
+                rhs=xq[c][:, a : a + n].bitcast(FP8X4),
+                rhs_scale=xqs[c][:, a : a + n],
                 start=True,
                 stop=True,
             )
-            nc.scalar.activation(out=hp[s][:, t, :n], in_=z[:, :n], func=RELU, bias=bias_h[:, g, t : t + 1])
+            nc.scalar.activation(out=hp[s][:, t, a : a + n], in_=z[:, :n], func=RELU, bias=bias_h[:, g, t : t + 1])
 
         def weave(move, s, a, b):
             if b > a:
@@ -229,13 +230,18 @@ def tile_spn_w4_kernel(tc, x_bytes, x_scale, w0_words, w0_scales, w1_words, w1_s
             nc.vector.tensor_tensor(out=res[:], in0=acc[last, j][:, 0, :], in1=bias_o[:], op=ADD)
             nc.sync.dma_start(out=out_view[:, first[last] + j, :], in_=res[:])
 
-        def spread_scales():
+        def spread_turn():
             spread = psum.tile([P, 4, P], F32, name="spread", tag="xo", bufs=3)
             for m in range(4):
                 nc.tensor.transpose(spread[:, m, :], xs_col[:, m : m + 1].to_broadcast([P, P]), ident[:])
-            nc.scalar.copy(out=xs[:].rearrange("p (n m) -> p n m", m=4), in_=spread[:].rearrange("p m n -> p n m"))
+            xt["scales"] = spread
+
+        def spread_copy():
+            nc.scalar.copy(out=xs[:].rearrange("p (n m) -> p n m", m=4), in_=xt["scales"][:].rearrange("p m n -> p n m"))
 
         def dummies(k):
+            if not k:
+                return
             d = psum.tile([P, 512], F32, name="z", bufs=5)
             for i in range(k):
                 nc.tensor.matmul(d[:], lhsT=zeros[:, :P], rhs=zeros[:], start=True, stop=True)
@@ -243,19 +249,24 @@ def tile_spn_w4_kernel(tc, x_bytes, x_scale, w0_words, w0_scales, w1_words, w1_s
         if WARM:
             dummies(WARM[0])
         for j in range(CHUNKS[0]):
-            x_cast(0, j, nc.vector.tensor_copy if j >= CHUNKS[0] - HEAD_V_CASTS else nc.scalar.copy)
+            x_cast(0, j, nc.vector.tensor_copy if j < HEAD_V_CASTS else nc.scalar.copy)
         permute_codes(0)
         pass
-        x_transpose(0, 0)
-        spread_scales()
+        x_transpose(0, 0, 1)
+        x_transpose(0, 1, 1)
+        spread_turn()
         if WARM:
             dummies(WARM[1])
         for j in range(CHUNKS[1]):
             x_cast(1, j, nc.scalar.copy)
-        permute_scales(0)
+        x_transpose(1, 0)
+        if WARM:
+            dummies(WARM[2])
+        spread_copy()
+        pass
         for j in range(CHUNKS[0]):
             x_scale_out(0, j)
-        pass
+        permute_scales(0)
         x_quantize(0)
         permute_codes(1)
         permute_scales(1)
@@ -294,15 +305,17 @@ def tile_spn_w4_kernel(tc, x_bytes, x_scale, w0_words, w0_scales, w1_words, w1_s
             c, g = units[s] if s < n_units else (n_chunks, 0)
             turn = HEAD_CHUNKS <= c + 1 < n_chunks and g == 1
             for t in range(4 if s < n_units else 1):
-                if s < n_units:
+                if s < n_units - 0:
                     plane(s, t)
+                elif s < n_units:
+                    plane(s, 2 * t % 4, t // 2 * P, P)
+                    plane(s, 2 * t % 4 + 1, t // 2 * P, P)
                 if t == 0:
                     if s > 0:
                         n1 = CHUNKS[units[s - 1][0]] * P
                         weave(nc.scalar.copy, s - 1, n1 - share(s - 1), n1)
-                    if s == 1:
-                        for pair in range(CHUNKS[1] // 2):
-                            x_transpose(1, pair)
+                if 4 * s + t == 4:
+                    x_transpose(1, 2)
                 if s < n_units:
                     for pair in range(2):
                         for u in range(s - 1):
@@ -311,7 +324,7 @@ def tile_spn_w4_kernel(tc, x_bytes, x_scale, w0_words, w0_scales, w1_words, w1_s
                                 stage2(u, (2 * pair, 2 * pair + 1))
             if turn:
                 for pair in range(CHUNKS[c + 1] // 2):
-                    x_transpose(c + 1, pair)
+                    x_transpose(c + 1, 2 * pair)
                     x_copy(c + 1, pair)
             if s == 0:
                 for gg in range(2, G):
@@ -327,7 +340,7 @@ def tile_spn_w4_kernel(tc, x_bytes, x_scale, w0_words, w0_scales, w1_words, w1_s
             if g == 2 and HEAD_CHUNKS <= c + 1 < n_chunks:
                 between.append((x_quantize, (c + 1,)))
             for cf in range(last):
-                pair = s - pass_plane(G * cf + G - 1) // 4 - (1 if cf < last - 1 else 0)
+                pair = s - pass_plane(G * cf + G - 1) // 4 - (1 if cf < last - 2 else 0 if cf < last - 1 else 0)
                 if 0 <= pair < CHUNKS[cf] // 2:
                     between.append((finish, (cf, pair)))
             cm, gm = divmod(s - 2, G)

@@ -24,9 +24,10 @@ FLOPS = 2 * B * X * N + 2 * B * H * OS
 
 CHUNKS = (2, 4, 4, 4, 2)
 HEAD_CHUNKS = 2
-SHARE_MID = (0,0,0,0)
-SHARE_HEAD = (0,0,0,0)
-SHARE_TAIL = (0,0,64,128)
+POOL_TOKENS = (256,384,384,256)
+SHARE = {15: 128, 18: 64}
+SHARE_AT = {15: 0, 18: 0}
+V_CASTS = (0, 0, 3, 3, 1)
 WARM = (5,1,0)
 HEAD_V_CASTS = 1
 
@@ -48,7 +49,6 @@ def tile_spn_w4_kernel(tc, x_bytes, x_scale, w0_words, w0_scales, w1_words, w1_s
         ctx.enter_context(tc.manual_schedule())
 
         ident = keep.tile([P, P], F32, name="ident")
-        xs = keep.tile([P, X], F32, name="xs")
         w0_raw = keep.tile([P, 2 * N], U8, name="w0_raw", align_bytes=64)
         w0s_raw = keep.tile([P, N], U8, name="w0s_raw", align_bytes=64)
         w0_perm = keep.tile([P, 2 * H], U8, name="w0_perm", align_bytes=64)
@@ -117,13 +117,8 @@ def tile_spn_w4_kernel(tc, x_bytes, x_scale, w0_words, w0_scales, w1_words, w1_s
                 in_=w0s_raw[:, 512 * g : 512 * (g + 1)].rearrange("p (m t) -> p t m", t=4),
             )
 
-        def x_mult(c, j):
-            t = work.tile([P, X], BF16, name="xv", bufs=8, align_bytes=64)
-            xv[c, j] = t
-            nc.vector.tensor_tensor(out=t[:], in0=xb[c][:, j, :].bitcast(FP8), in1=xs[:], op=MULT)
-
         def x_cast(c, j, move):
-            t = work.tile([P, X], BF16, name="xv", bufs=8, align_bytes=64)
+            t = work.tile([P, X], BF16, name="xv", bufs=12, align_bytes=64)
             xv[c, j] = t
             move(out=t[:], in_=xb[c][:, j, :].bitcast(FP8))
 
@@ -145,30 +140,17 @@ def tile_spn_w4_kernel(tc, x_bytes, x_scale, w0_words, w0_scales, w1_words, w1_s
                 op=MULT,
             )
 
-        def x_copy(c, pair):
-            if pair == 0:
-                xg[c] = work.tile([P, 2048], BF16, name="xg", bufs=2, align_bytes=64)
-            nc.scalar.copy(
-                out=xg[c][:, 1024 * pair : 1024 * (pair + 1)].bitcast(F32).rearrange("p (j r u) -> p j r u", j=2, u=2),
-                in_=xt[c, 2 * pair][0][:].rearrange("p j u r -> p j r u"),
-            )
-
         def x_quantize(c):
             n = CHUNKS[c] * P
             xq[c] = work.tile([P, 512], U32, name="xq", bufs=n_chunks, align_bytes=64)
             xqs[c] = work.tile([P, 512], U8, name="xqs", bufs=n_chunks, align_bytes=64)
             nc.vector.quantize_mx(out=xq[c][:, :n].bitcast(FP8X4), scales=xqs[c][:, :n], in_=xg[c][:, : 4 * n])
 
-        def share(s):
-            c, g = units[s]
-            return SHARE_HEAD[g] if c == 0 else SHARE_TAIL[g] if c == last else SHARE_MID[g] if c < 3 else 0
-
         def plane(s, t, a=0, n=None):
             c, g = units[s]
             n = n or CHUNKS[c] * P
             if t == 0 and a == 0:
                 hp[s] = work.tile([P, 4, 512], BF16, name="hp", bufs=6, align_bytes=64)
-                hg[s] = work.tile([P, 2048], BF16, name="hg", bufs=6, align_bytes=64)
             z = psum.tile([P, 512], F32, name="z", bufs=5)
             m0 = 512 * g + P * t
             nc.tensor.matmul_mx(
@@ -182,18 +164,35 @@ def tile_spn_w4_kernel(tc, x_bytes, x_scale, w0_words, w0_scales, w1_words, w1_s
             )
             nc.scalar.activation(out=hp[s][:, t, a : a + n], in_=z[:, :n], func=RELU, bias=bias_h[:, g, t : t + 1])
 
-        def weave(move, s, a, b):
-            if b > a:
+        def pool_copy(out, in_):
+            nc.gpsimd.tensor_scalar(out=out, in0=in_, scalar1=1.0, scalar2=0.0, op0=MULT, op1=ADD)
+
+        def weave(move, s, a, b, tag="hg", bufs=4):
+            if (s, a) not in hg:
+                hg[s, a] = work.tile([P, 4 * (b - a)], BF16, name="hg", tag=tag, bufs=bufs, align_bytes=64)
+            if move is pool_copy:
+                move(out=hg[s, a][:].rearrange("p (n t) -> p n t", t=4), in_=hp[s][:, :, a:b].rearrange("p t n -> p n t"))
+            else:
+                e = b - SHARE.get(s, 0) * (b == tokens(s))
                 move(
-                    out=hg[s][:, 4 * a : 4 * b].rearrange("p (c i t) -> p c t i", t=4, i=4),
-                    in_=hp[s][:, :, a:b].rearrange("p t (c i) -> p c t i", i=4),
+                    out=hg[s, a][:, : 4 * (e - a)].rearrange("p (c i t) -> p c t i", t=4, i=4),
+                    in_=hp[s][:, :, a:e].rearrange("p t (c i) -> p c t i", i=4),
                 )
 
+        def scalar_share(s, a):
+            b = tokens(s)
+            e = b - SHARE[s]
+            hg[s, a] = work.tile([P, 4 * (b - a)], BF16, name="hg", tag="hs", bufs=3, align_bytes=64)
+            nc.scalar.copy(
+                out=hg[s, a][:, 4 * (e - a) :].rearrange("p (c i t) -> p c t i", t=4, i=4),
+                in_=hp[s][:, :, e:b].rearrange("p t (c i) -> p c t i", i=4),
+            )
+
         def h_quantize(s, a, b):
-            if a == 0:
+            if s not in hq:
                 hq[s] = work.tile([P, 512], U32, name="hq", bufs=12, align_bytes=64)
                 hqs[s] = work.tile([P, 512], U8, name="hqs", bufs=12, align_bytes=64)
-            nc.vector.quantize_mx(out=hq[s][:, a:b].bitcast(FP8X4), scales=hqs[s][:, a:b], in_=hg[s][:, 4 * a : 4 * b])
+            nc.vector.quantize_mx(out=hq[s][:, a:b].bitcast(FP8X4), scales=hqs[s][:, a:b], in_=hg[s, a][:])
 
         def out_pass(dst, lhs, lhs_scales, j, rhs, rhs_scales, start, stop):
             cols = slice(j * P, (j + 1) * P)
@@ -230,15 +229,6 @@ def tile_spn_w4_kernel(tc, x_bytes, x_scale, w0_words, w0_scales, w1_words, w1_s
             nc.vector.tensor_tensor(out=res[:], in0=acc[last, j][:, 0, :], in1=bias_o[:], op=ADD)
             nc.sync.dma_start(out=out_view[:, first[last] + j, :], in_=res[:])
 
-        def spread_turn():
-            spread = psum.tile([P, 4, P], F32, name="spread", tag="xo", bufs=3)
-            for m in range(4):
-                nc.tensor.transpose(spread[:, m, :], xs_col[:, m : m + 1].to_broadcast([P, P]), ident[:])
-            xt["scales"] = spread
-
-        def spread_copy():
-            nc.scalar.copy(out=xs[:].rearrange("p (n m) -> p n m", m=4), in_=xt["scales"][:].rearrange("p m n -> p n m"))
-
         def dummies(k):
             if not k:
                 return
@@ -251,10 +241,8 @@ def tile_spn_w4_kernel(tc, x_bytes, x_scale, w0_words, w0_scales, w1_words, w1_s
         for j in range(CHUNKS[0]):
             x_cast(0, j, nc.vector.tensor_copy if j < HEAD_V_CASTS else nc.scalar.copy)
         permute_codes(0)
-        pass
         x_transpose(0, 0, 1)
         x_transpose(0, 1, 1)
-        spread_turn()
         if WARM:
             dummies(WARM[1])
         for j in range(CHUNKS[1]):
@@ -262,7 +250,6 @@ def tile_spn_w4_kernel(tc, x_bytes, x_scale, w0_words, w0_scales, w1_words, w1_s
         x_transpose(1, 0)
         if WARM:
             dummies(WARM[2])
-        spread_copy()
         pass
         for j in range(CHUNKS[0]):
             x_scale_out(0, j)
@@ -271,85 +258,94 @@ def tile_spn_w4_kernel(tc, x_bytes, x_scale, w0_words, w0_scales, w1_words, w1_s
         permute_codes(1)
         permute_scales(1)
 
-        waiting = []
+        def tokens(u):
+            return CHUNKS[units[u][0]] * P
 
-        def vector_step(s, between):
-            n = CHUNKS[units[s][0]] * P
-            end = n - share(s)
-            cuts = (0, n // 2, n) if s == n_units - 1 or (not between and not waiting and s >= 15) else (0, n)
-            for a, b in zip(cuts, cuts[1:]):
-                weave(nc.vector.tensor_copy, s, a, min(b, end))
-            if waiting:
-                between = [(h_quantize, waiting.pop())] + between
-            elif not between and len(cuts) == 2:
-                waiting.append((s, 0, n))
-                return
-            for f, args in between:
-                f(*args)
-            for a, b in zip(cuts, cuts[1:]):
-                h_quantize(s, a, b)
+        def whole_stage2(c, pair):
+            for g in range(G):
+                stage2(G * c + g, (2 * pair, 2 * pair + 1))
 
-        widths = [CHUNKS[c] * P for c, g in units for t in range(4)]
+        def v_casts(c, lo, hi):
+            for j in range(CHUNKS[c] - V_CASTS[c], CHUNKS[c]):
+                if lo <= j - (CHUNKS[c] - V_CASTS[c]) < hi:
+                    x_cast(c, j, nc.vector.tensor_copy)
 
-        def pass_plane(u):
-            c = units[u][0]
-            u = max(u, G * c + (G - 1 if c < last - 1 else 1 if c < last else 0))
-            k = 4 * (u + 1)
-            ahead = 0
-            while k < len(widths) and ahead < (3072 if c < last - 2 else 2048 if c < last - 1 else 1536):
-                ahead = ahead + widths[k]
-                k = k + 1
-            return min(k + 5 - 1, len(widths) - 1)
+        def vector_step(u):
+            c, g = units[u]
+            n = tokens(u)
+            if g == 0 and c < last:
+                cut = n - POOL_TOKENS[c]
+                if c > 0:
+                    h_quantize(u - 1, 0, tokens(u - 1))
+                    whole_stage2(c - 1, 0)
+                if cut:
+                    weave(nc.vector.tensor_copy, u, 0, cut)
+                if cut < n:
+                    weave(pool_copy, u, cut, n, "hand", 1)
+                for j in range(CHUNKS[c + 1]):
+                    x_scale_out(c + 1, j)
+                if c > 0:
+                    finish(c - 1, 0)
+                if cut:
+                    h_quantize(u, 0, cut)
+                x_quantize(c + 1)
+                if cut < n:
+                    h_quantize(u, cut, n)
+            elif g == G - 1 and c + 1 < last:
+                weave(nc.vector.tensor_copy, u, 0, n, "hand", 1)
+                if c + 3 < n_chunks:
+                    v_casts(c + 3, 0, 4)
+                if 3 == G - 1 and c > 0 and CHUNKS[c - 1] > 2:
+                    finish(c - 1, 1)
+            elif u == n_units - 1:
+                weave(nc.vector.tensor_copy, u, 0, P)
+                weave(nc.scalar.copy, u, P, n)
+                h_quantize(u, 0, P)
+                h_quantize(u, P, n)
+            else:
+                between = []
+                if g == 3 and 0 < c < last and CHUNKS[c - 1] > 2:
+                    between.append((finish, (c - 1, 1)))
+                if c == last and g - 1 in (0, 1):
+                    between.append((finish, (c - 1, g - 1)))
+                if g in (1, 1 + 1) and c == 0 and V_CASTS[c + 2] > 2 * (g - 1):
+                    between.append((v_casts, (c + 2, 2 * (g - 1), 2 * (g - 1) + 2)))
+                cuts = (0, n) if between else (0, n // 2, n)
+                if c == last and g >= 9:
+                    cuts = (0, n // 2, n)
+                for a, b in zip(cuts, cuts[1:]):
+                    weave(nc.scalar.copy if c == last and g >= 9 and a else nc.vector.tensor_copy, u, a, b)
+                for f, args in between:
+                    f(*args)
+                for a, b in zip(cuts, cuts[1:]):
+                    h_quantize(u, a, b)
 
-        for s in range(n_units + 1):
-            c, g = units[s] if s < n_units else (n_chunks, 0)
-            turn = HEAD_CHUNKS <= c + 1 < n_chunks and g == 1
-            for t in range(4 if s < n_units else 1):
-                if s < n_units - 0:
-                    plane(s, t)
-                elif s < n_units:
-                    plane(s, 2 * t % 4, t // 2 * P, P)
-                    plane(s, 2 * t % 4 + 1, t // 2 * P, P)
-                if t == 0:
-                    if s > 0:
-                        n1 = CHUNKS[units[s - 1][0]] * P
-                        weave(nc.scalar.copy, s - 1, n1 - share(s - 1), n1)
-                if 4 * s + t == 4:
-                    x_transpose(1, 2)
-                if s < n_units:
-                    for pair in range(2):
-                        for u in range(s - 1):
-                            cu = units[u][0]
-                            if 2 * pair < CHUNKS[cu] and pass_plane(u) + (4 * pair if cu < last - 1 else 0) == 4 * s + t:
-                                stage2(u, (2 * pair, 2 * pair + 1))
-            if turn:
+        n_planes = 4 * n_units
+        for k in range(n_planes + 4 + 2):
+            s, t = divmod(k, 4)
+            c, g = divmod(s, G)
+            if k < n_planes:
+                plane(s, t)
+            if t == 0 and s - 1 in SHARE:
+                scalar_share(s - 1, SHARE_AT[s - 1])
+            if k == 4:
+                x_transpose(1, 2)
+            if g == 3 and HEAD_CHUNKS <= c + 2 < n_chunks and t < CHUNKS[c + 2] - V_CASTS[c + 2]:
+                x_cast(c + 2, t, nc.scalar.copy)
+            if k % 16 == 2 and HEAD_CHUNKS <= c + 1 < n_chunks:
                 for pair in range(CHUNKS[c + 1] // 2):
                     x_transpose(c + 1, 2 * pair)
-                    x_copy(c + 1, pair)
-            if s == 0:
+            if k % 16 == 12 and 0 < c < last and CHUNKS[c - 1] > 2:
+                whole_stage2(c - 1, 1)
+            for u in range(G * (last - 1), n_units - 1):
+                if k == max(4 * u + 13, 4 * G * (last - 1) + 15):
+                    stage2(u, range(CHUNKS[units[u][0]]))
+            if k == 3:
                 for gg in range(2, G):
                     permute_codes(gg)
                     permute_scales(gg)
-                continue
-            between = []
-            if s == 1:
-                for j in range(CHUNKS[1]):
-                    x_scale_out(1, j)
-            if s == 1:
-                between.append((x_quantize, (1,)))
-            if g == 2 and HEAD_CHUNKS <= c + 1 < n_chunks:
-                between.append((x_quantize, (c + 1,)))
-            for cf in range(last):
-                pair = s - pass_plane(G * cf + G - 1) // 4 - (1 if cf < last - 2 else 0 if cf < last - 1 else 0)
-                if 0 <= pair < CHUNKS[cf] // 2:
-                    between.append((finish, (cf, pair)))
-            cm, gm = divmod(s - 2, G)
-            if HEAD_CHUNKS <= cm + 2 < n_chunks:
-                for j in range(2 * gm, min(2 * gm + 2, CHUNKS[cm + 2])):
-                    between.append((x_mult, (cm + 2, j)))
-            vector_step(s - 1, between)
-            if s == n_units - 1:
-                stage2(s - 1, range(CHUNKS[last]))
+            if k >= 7 + 2 and (k - 2) % 4 == 3:
+                vector_step((k - 2) // 4 - 1)
         for j in range(CHUNKS[last]):
             stage2(n_units - 1, (j,))
             finish_last(j)

@@ -25,10 +25,10 @@ FLOPS = 2 * B * X * N + 2 * B * H * OS
 CHUNKS = (2, 4, 4, 4, 2)
 HEAD_CHUNKS = 2
 POOL_TOKENS = (256,384,384,256)
-SHARE = {15: 128, 18: 64}
-SHARE_AT = {15: 0, 18: 0}
-V_CASTS = (0, 0, 3, 3, 1)
-WARM = (5,1,0)
+SHARE = {15: 128, 16: 64}
+SHARE_AT = {15: 0, 16: 0}
+V_CASTS = (0, 0, 1, 4, 2)
+WARM = (5, 1, 0)
 HEAD_V_CASTS = 1
 
 
@@ -79,19 +79,19 @@ def tile_spn_w4_kernel(tc, x_bytes, x_scale, w0_words, w0_scales, w1_words, w1_s
         if WARM:
             nc.scalar.activation(out=warm[:], in_=warm[:], func=RELU)
         load_x(0)
-        nc.sync.dma_start(out=w0_raw[:, 0:1024], in_=w0_words[0, :, 0:1024])
         nc.sync.dma_start(out=xs_col[:], in_=x_scale.rearrange("o (n m) -> n (o m)", m=4))
         load_x(1)
+        nc.sync.dma_start(out=w0_raw[:, 0:1024], in_=w0_words[0, :, 0:1024])
         for q in range(4):
             nc.sync.dma_start(
                 out=w0s_raw[32 * q : 32 * q + 4, :].bitcast(I32),
                 in_=w0_scales[0, 4 * q : 4 * q + 4, :].bitcast(I32),
             )
-        pass
+        load_x(2)
         nc.sync.dma_start(out=bias_h[:], in_=biases[0:H].rearrange("(g p t) -> p g t", g=G, p=P, t=4))
         nc.sync.dma_start(out=w0_raw[:, 1024:2048], in_=w0_words[0, :, 1024:2048])
+        pass
         nc.sync.dma_start(out=w0_raw[:, 2048:4608], in_=w0_words[0, :, 2048:4608])
-        load_x(2)
         nc.sync.dma_start(out=w1[:], in_=w1_words.rearrange("g p n -> p g n"))
         for q in range(4):
             nc.sync.dma_start(
@@ -238,21 +238,23 @@ def tile_spn_w4_kernel(tc, x_bytes, x_scale, w0_words, w0_scales, w1_words, w1_s
 
         if WARM:
             dummies(WARM[0])
-        for j in range(CHUNKS[0]):
-            x_cast(0, j, nc.vector.tensor_copy if j < HEAD_V_CASTS else nc.scalar.copy)
-        permute_codes(0)
+        x_cast(0, 0, nc.vector.tensor_copy)
+        x_cast(0, 1, nc.scalar.copy)
         x_transpose(0, 0, 1)
         x_transpose(0, 1, 1)
-        if WARM:
-            dummies(WARM[1])
         for j in range(CHUNKS[1]):
-            x_cast(1, j, nc.scalar.copy)
+            x_cast(1, j, nc.vector.tensor_copy if j < 2 else nc.scalar.copy)
         x_transpose(1, 0)
         if WARM:
-            dummies(WARM[2])
-        pass
+            dummies(WARM[1])
         for j in range(CHUNKS[0]):
             x_scale_out(0, j)
+        x_transpose(1, 2)
+        if WARM:
+            dummies(WARM[2])
+        for j in range(2):
+            x_cast(2, j, nc.scalar.copy)
+        permute_codes(0)
         permute_scales(0)
         x_quantize(0)
         permute_codes(1)
@@ -291,34 +293,32 @@ def tile_spn_w4_kernel(tc, x_bytes, x_scale, w0_words, w0_scales, w1_words, w1_s
                 x_quantize(c + 1)
                 if cut < n:
                     h_quantize(u, cut, n)
-            elif g == G - 1 and c + 1 < last:
-                weave(nc.vector.tensor_copy, u, 0, n, "hand", 1)
-                if c + 3 < n_chunks:
-                    v_casts(c + 3, 0, 4)
-                if 3 == G - 1 and c > 0 and CHUNKS[c - 1] > 2:
-                    finish(c - 1, 1)
-            elif u == n_units - 1:
+                return
+            if u == n_units - 1:
                 weave(nc.vector.tensor_copy, u, 0, P)
                 weave(nc.scalar.copy, u, P, n)
+                h_quantize(u - 1, 0, tokens(u - 1))
+                stage2(u - 1, range(CHUNKS[last]))
                 h_quantize(u, 0, P)
                 h_quantize(u, P, n)
+                finish(last - 1, 1)
+                return
+            if g == G - 1 and c + 1 < last:
+                weave(nc.vector.tensor_copy, u, 0, n, "hand", 1)
             else:
-                between = []
-                if g == 3 and 0 < c < last and CHUNKS[c - 1] > 2:
-                    between.append((finish, (c - 1, 1)))
-                if c == last and g - 1 in (0, 1):
-                    between.append((finish, (c - 1, g - 1)))
-                if g in (1, 1 + 1) and c == 0 and V_CASTS[c + 2] > 2 * (g - 1):
-                    between.append((v_casts, (c + 2, 2 * (g - 1), 2 * (g - 1) + 2)))
-                cuts = (0, n) if between else (0, n // 2, n)
-                if c == last and g >= 9:
-                    cuts = (0, n // 2, n)
-                for a, b in zip(cuts, cuts[1:]):
-                    weave(nc.scalar.copy if c == last and g >= 9 and a else nc.vector.tensor_copy, u, a, b)
-                for f, args in between:
-                    f(*args)
-                for a, b in zip(cuts, cuts[1:]):
-                    h_quantize(u, a, b)
+                weave(nc.vector.tensor_copy, u, 0, n)
+            if (g > 1 or c == last) and u != G * last:
+                h_quantize(u - 1, 0, tokens(u - 1))
+            if u == G * last - 1:
+                h_quantize(u, 0, n)
+            if g == 3 and 0 < c < last and CHUNKS[c - 1] > 2:
+                finish(c - 1, 1)
+            if u == G * last + 1:
+                finish(last - 1, 0)
+            if c == 0 and g < G - 1:
+                v_casts(2, 2 * (g - 1), 2 * g)
+            if g == G - 1 and c + 3 < n_chunks:
+                v_casts(c + 3, 0, 4)
 
         n_planes = 4 * n_units
         for k in range(n_planes + 4 + 2):
@@ -328,17 +328,15 @@ def tile_spn_w4_kernel(tc, x_bytes, x_scale, w0_words, w0_scales, w1_words, w1_s
                 plane(s, t)
             if t == 0 and s - 1 in SHARE:
                 scalar_share(s - 1, SHARE_AT[s - 1])
-            if k == 4:
-                x_transpose(1, 2)
-            if g == 3 and HEAD_CHUNKS <= c + 2 < n_chunks and t < CHUNKS[c + 2] - V_CASTS[c + 2]:
+            if g == 3 and HEAD_CHUNKS <= c + 2 < n_chunks and (2 if c == 0 else 0) <= t < CHUNKS[c + 2] - V_CASTS[c + 2]:
                 x_cast(c + 2, t, nc.scalar.copy)
             if k % 16 == 2 and HEAD_CHUNKS <= c + 1 < n_chunks:
                 for pair in range(CHUNKS[c + 1] // 2):
                     x_transpose(c + 1, 2 * pair)
             if k % 16 == 12 and 0 < c < last and CHUNKS[c - 1] > 2:
                 whole_stage2(c - 1, 1)
-            for u in range(G * (last - 1), n_units - 1):
-                if k == max(4 * u + 13, 4 * G * (last - 1) + 15):
+            for u in range(G * (last - 1), n_units - 2):
+                if k == min(max(4 * u + 17, 4 * G * (last - 1) + 17), n_planes + 2):
                     stage2(u, range(CHUNKS[units[u][0]]))
             if k == 3:
                 for gg in range(2, G):

@@ -15,6 +15,7 @@ FP4X4 = mybir.dt.float4_e2m1fn_x4
 RELU = mybir.ActivationFunctionType.Relu
 MULT = mybir.AluOpType.mult
 ADD = mybir.AluOpType.add
+MAX = mybir.AluOpType.max
 
 P = 128
 B, X, N, OS = 2048, 512, 2304, 256
@@ -24,10 +25,10 @@ FLOPS = 2 * B * X * N + 2 * B * H * OS
 
 CHUNKS = (2, 4, 4, 4, 2)
 HEAD_CHUNKS = 2
+V_PLANES = (11,)
 POOL_TOKENS = (256,384,384,256)
-SHARE = {15: 128, 16: 64}
+SHARE = {15: 128, 16: 128}
 SHARE_AT = {15: 0, 16: 0}
-V_CASTS = (0, 0, 1, 4, 2)
 WARM = (5, 1, 0)
 HEAD_V_CASTS = 1
 
@@ -103,40 +104,48 @@ def tile_spn_w4_kernel(tc, x_bytes, x_scale, w0_words, w0_scales, w1_words, w1_s
         nc.sync.dma_start(out=bias_o[:], in_=biases[H:N].partition_broadcast(P))
 
         xv, xt, xg, xq, xqs = {}, {}, {}, {}, {}
+        held = {}
         hp, hg, hq, hqs, acc = {}, {}, {}, {}, {}
 
-        def permute_codes(g):
+        taken = []
+
+        def side_bank():
+            taken.append(len(taken) % 3)
+            return "side%d" % taken[-1]
+
+        def permute_codes(g0, g1):
             nc.vector.tensor_copy(
-                out=w0_perm[:, 1024 * g : 1024 * (g + 1)].bitcast(U16).rearrange("p (t m) -> p t m", t=4),
-                in_=w0_raw[:, 1024 * g : 1024 * (g + 1)].bitcast(U16).rearrange("p (m t) -> p t m", t=4),
+                out=w0_perm[:, 1024 * g0 : 1024 * g1].bitcast(U16).rearrange("p (g t m) -> p g t m", t=4, m=P),
+                in_=w0_raw[:, 1024 * g0 : 1024 * g1].bitcast(U16).rearrange("p (g m t) -> p g t m", t=4, m=P),
             )
 
-        def permute_scales(g):
+        def permute_scales(g0, g1):
             nc.vector.tensor_copy(
-                out=w0s_perm[:, 512 * g : 512 * (g + 1)].rearrange("p (t m) -> p t m", t=4),
-                in_=w0s_raw[:, 512 * g : 512 * (g + 1)].rearrange("p (m t) -> p t m", t=4),
+                out=w0s_perm[:, 512 * g0 : 512 * g1].rearrange("p (g t m) -> p g t m", t=4, m=P),
+                in_=w0s_raw[:, 512 * g0 : 512 * g1].rearrange("p (g m t) -> p g t m", t=4, m=P),
             )
 
-        def x_cast(c, j, move):
-            t = work.tile([P, X], BF16, name="xv", bufs=12, align_bytes=64)
-            xv[c, j] = t
-            move(out=t[:], in_=xb[c][:, j, :].bitcast(FP8))
+        def x_cast(c, j0, count, move):
+            t = work.tile([P, count, X], BF16, name="xv", tag="xv%d" % count, bufs=8 // count, align_bytes=64)
+            for jj in range(count):
+                xv[c, j0 + jj] = t[:, jj, :]
+            move(out=t[:].rearrange("p j k -> p (j k)"), in_=xb[c][:, j0 : j0 + count, :].rearrange("p j k -> p (j k)").bitcast(FP8))
 
         def x_transpose(c, j0, count=2):
-            t = psum.tile([P, count, 2, P], F32, name="xt", tag="xo", bufs=3)
+            t = psum.tile([P, 2, count, P], F32, name="xt", tag=side_bank(), bufs=1)
+            xt[c, j0] = t
             for jj in range(count):
-                xt[c, j0 + jj] = (t, jj)
-                words = xv[c, j0 + jj][:].bitcast(F32)
+                words = xv[c, j0 + jj].bitcast(F32)
                 for u in range(2):
-                    nc.tensor.transpose(t[:, jj, u, :], words[:, u : X // 2 : 2], ident[:])
+                    nc.tensor.transpose(t[:, u, jj, :], words[:, u : X // 2 : 2], ident[:])
 
-        def x_scale_out(c, j):
-            if j == 0:
+        def x_scale_out(c, j0, count=2):
+            if j0 == 0:
                 xg[c] = work.tile([P, 2048], BF16, name="xg", bufs=2, align_bytes=64)
             nc.vector.tensor_tensor(
-                out=xg[c][:, 512 * j : 512 * (j + 1)].rearrange("p (r u e) -> p r u e", u=2, e=2),
-                in0=xt[c, j][0][:, xt[c, j][1]].rearrange("p u r -> p (u r)").bitcast(BF16).rearrange("p (u r e) -> p r u e", u=2, e=2),
-                in1=xs_col[:].rearrange("p (o u e) -> p o u e", o=1, u=2).to_broadcast([P, P, 2, 2]),
+                out=xg[c][:, 512 * j0 : 512 * (j0 + count)].rearrange("p (r u e) -> p r u e", u=2, e=2),
+                in0=xt[c, j0][:].rearrange("p u j r -> p (u j r)").bitcast(BF16).rearrange("p (u r e) -> p r u e", u=2, e=2),
+                in1=xs_col[:].rearrange("p (o u e) -> p o u e", o=1, u=2).to_broadcast([P, count * P, 2, 2]),
                 op=MULT,
             )
 
@@ -162,7 +171,16 @@ def tile_spn_w4_kernel(tc, x_bytes, x_scale, w0_words, w0_scales, w1_words, w1_s
                 start=True,
                 stop=True,
             )
-            nc.scalar.activation(out=hp[s][:, t, a : a + n], in_=z[:, :n], func=RELU, bias=bias_h[:, g, t : t + 1])
+            if 4 * s + t in V_PLANES:
+                held[4 * s + t] = z
+            else:
+                nc.scalar.activation(out=hp[s][:, t, a : a + n], in_=z[:, :n], func=RELU, bias=bias_h[:, g, t : t + 1])
+
+        def v_plane(k):
+            s, t = divmod(k, 4)
+            c, g = units[s]
+            n = CHUNKS[c] * P
+            nc.vector.tensor_scalar(out=hp[s][:, t, :n], in0=held[k][:, :n], scalar1=bias_h[:, g, t : t + 1], scalar2=0.0, op0=ADD, op1=MAX)
 
         def pool_copy(out, in_):
             nc.gpsimd.tensor_scalar(out=out, in0=in_, scalar1=1.0, scalar2=0.0, op0=MULT, op1=ADD)
@@ -212,7 +230,7 @@ def tile_spn_w4_kernel(tc, x_bytes, x_scale, w0_words, w0_scales, w1_words, w1_s
             for j in tiles:
                 if g == 0:
                     if j % per_bank == 0:
-                        tag, bufs = ("xo", 3) if c < last or j == 0 else ("z", 5)
+                        tag, bufs = (side_bank(), 1) if c < last or j == 0 else ("z", 5)
                         acc[c, j // per_bank] = psum.tile([P, per_bank, OS], F32, name="o", tag=tag, bufs=bufs)
                     out_pass(acc[c, j // per_bank][:, j % per_bank, :], xq[c], xqs[c], j, w0_raw[:, 2 * H : 2 * N], w0s_raw[:, H:N], j % per_bank == 0, False)
                 closes = g == G - 1 and j % per_bank == per_bank - 1
@@ -238,27 +256,27 @@ def tile_spn_w4_kernel(tc, x_bytes, x_scale, w0_words, w0_scales, w1_words, w1_s
 
         if WARM:
             dummies(WARM[0])
-        x_cast(0, 0, nc.vector.tensor_copy)
-        x_cast(0, 1, nc.scalar.copy)
+        x_cast(0, 0, 1, nc.vector.tensor_copy)
+        x_cast(0, 1, 1, nc.scalar.copy)
         x_transpose(0, 0, 1)
         x_transpose(0, 1, 1)
-        for j in range(CHUNKS[1]):
-            x_cast(1, j, nc.vector.tensor_copy if j < 2 else nc.scalar.copy)
+        x_cast(1, 0, 1, nc.vector.tensor_copy)
+        for j in range(1, CHUNKS[1]):
+            x_cast(1, j, 1, nc.scalar.copy)
+        permute_codes(0, 1)
         x_transpose(1, 0)
         if WARM:
             dummies(WARM[1])
         for j in range(CHUNKS[0]):
-            x_scale_out(0, j)
+            x_scale_out(0, j, 1)
         x_transpose(1, 2)
-        if WARM:
-            dummies(WARM[2])
-        for j in range(2):
-            x_cast(2, j, nc.scalar.copy)
-        permute_codes(0)
-        permute_scales(0)
+        x_cast(2, 0, 2, nc.scalar.copy)
+        permute_scales(0, 1)
         x_quantize(0)
-        permute_codes(1)
-        permute_scales(1)
+        permute_scales(1, 2)
+        permute_codes(1, 2)
+        permute_scales(2, G)
+        permute_codes(2, G)
 
         def tokens(u):
             return CHUNKS[units[u][0]] * P
@@ -266,11 +284,6 @@ def tile_spn_w4_kernel(tc, x_bytes, x_scale, w0_words, w0_scales, w1_words, w1_s
         def whole_stage2(c, pair):
             for g in range(G):
                 stage2(G * c + g, (2 * pair, 2 * pair + 1))
-
-        def v_casts(c, lo, hi):
-            for j in range(CHUNKS[c] - V_CASTS[c], CHUNKS[c]):
-                if lo <= j - (CHUNKS[c] - V_CASTS[c]) < hi:
-                    x_cast(c, j, nc.vector.tensor_copy)
 
         def vector_step(u):
             c, g = units[u]
@@ -284,28 +297,55 @@ def tile_spn_w4_kernel(tc, x_bytes, x_scale, w0_words, w0_scales, w1_words, w1_s
                     weave(nc.vector.tensor_copy, u, 0, cut)
                 if cut < n:
                     weave(pool_copy, u, cut, n, "hand", 1)
-                for j in range(CHUNKS[c + 1]):
+                for j in range(0, CHUNKS[c + 1], 2):
                     x_scale_out(c + 1, j)
                 if c > 0:
                     finish(c - 1, 0)
+                return
+            rest_of_step(u)
+
+        def window_end(u):
+                c, g = units[u]
+                n = tokens(u)
+                cut = n - POOL_TOKENS[c]
+                for k in V_PLANES:
+                    if k // 16 == c:
+                        v_plane(k)
                 if cut:
                     h_quantize(u, 0, cut)
                 x_quantize(c + 1)
                 if cut < n:
                     h_quantize(u, cut, n)
-                return
+
+        def rest_of_step(u):
+            c, g = units[u]
+            n = tokens(u)
             if u == n_units - 1:
-                weave(nc.vector.tensor_copy, u, 0, P)
-                weave(nc.scalar.copy, u, P, n)
-                h_quantize(u - 1, 0, tokens(u - 1))
-                stage2(u - 1, range(CHUNKS[last]))
-                h_quantize(u, 0, P)
-                h_quantize(u, P, n)
-                finish(last - 1, 1)
+                def wa():
+                    weave(nc.vector.tensor_copy, u, 0, P)
+                def wb():
+                    weave(nc.scalar.copy, u, P, n)
+                def qp():
+                    h_quantize(u - 1, 0, tokens(u - 1))
+                    stage2(u - 1, range(CHUNKS[last]))
+                def qa():
+                    h_quantize(u, 0, P)
+                    stage2(u, (0,))
+                def qb():
+                    h_quantize(u, P, n)
+                    stage2(u, (1,))
+                def f3():
+                    finish(last - 1, 1)
+                def fa():
+                    finish_last(0)
+                def fb():
+                    finish_last(1)
+                for f in (wa, wb, qp, qa, qb, f3, fa, fb):
+                    f()
                 return
             if g == G - 1 and c + 1 < last:
                 weave(nc.vector.tensor_copy, u, 0, n, "hand", 1)
-            else:
+            elif (u, 0) not in hg or u in SHARE:
                 weave(nc.vector.tensor_copy, u, 0, n)
             if (g > 1 or c == last) and u != G * last:
                 h_quantize(u - 1, 0, tokens(u - 1))
@@ -315,35 +355,33 @@ def tile_spn_w4_kernel(tc, x_bytes, x_scale, w0_words, w0_scales, w1_words, w1_s
                 finish(c - 1, 1)
             if u == G * last + 1:
                 finish(last - 1, 0)
-            if c == 0 and g < G - 1:
-                v_casts(2, 2 * (g - 1), 2 * g)
+            if u == 1 and 1:
+                x_cast(2, 4 - 1, 1, nc.vector.tensor_copy)
             if g == G - 1 and c + 3 < n_chunks:
-                v_casts(c + 3, 0, 4)
+                x_cast(c + 3, 0, CHUNKS[c + 3], nc.vector.tensor_copy)
 
         n_planes = 4 * n_units
         for k in range(n_planes + 4 + 2):
             s, t = divmod(k, 4)
             c, g = divmod(s, G)
-            if k < n_planes:
+            if k < n_planes - 4 * 0:
                 plane(s, t)
+            elif k < n_planes:
+                plane(s, 2 * t % 4, t // 2 * P, P)
+                plane(s, 2 * t % 4 + 1, t // 2 * P, P)
             if t == 0 and s - 1 in SHARE:
                 scalar_share(s - 1, SHARE_AT[s - 1])
-            if g == 3 and HEAD_CHUNKS <= c + 2 < n_chunks and (2 if c == 0 else 0) <= t < CHUNKS[c + 2] - V_CASTS[c + 2]:
-                x_cast(c + 2, t, nc.scalar.copy)
+            if k == 14 and 1 < 2:
+                x_cast(2, 2, 2 - 1, nc.scalar.copy)
             if k % 16 == 2 and HEAD_CHUNKS <= c + 1 < n_chunks:
                 for pair in range(CHUNKS[c + 1] // 2):
                     x_transpose(c + 1, 2 * pair)
-            if k % 16 == 12 and 0 < c < last and CHUNKS[c - 1] > 2:
+            if k % 16 == 13 and 0 < c < last and CHUNKS[c - 1] > 2:
                 whole_stage2(c - 1, 1)
             for u in range(G * (last - 1), n_units - 2):
                 if k == min(max(4 * u + 17, 4 * G * (last - 1) + 17), n_planes + 2):
                     stage2(u, range(CHUNKS[units[u][0]]))
-            if k == 3:
-                for gg in range(2, G):
-                    permute_codes(gg)
-                    permute_scales(gg)
             if k >= 7 + 2 and (k - 2) % 4 == 3:
                 vector_step((k - 2) // 4 - 1)
-        for j in range(CHUNKS[last]):
-            stage2(n_units - 1, (j,))
-            finish_last(j)
+            if k // 16 < last and k % 16 == max([7 + 2] + [v % 16 for v in V_PLANES if v // 16 == k // 16]):
+                window_end(k // 16 * G)

@@ -13,6 +13,7 @@ FP8 = mybir.dt.float8_e4m3fn
 FP8X4 = mybir.dt.float8_e4m3fn_x4
 FP4X4 = mybir.dt.float4_e2m1fn_x4
 RELU = mybir.ActivationFunctionType.Relu
+COPY = mybir.ActivationFunctionType.Copy
 MULT = mybir.AluOpType.mult
 ADD = mybir.AluOpType.add
 MAX = mybir.AluOpType.max
@@ -29,7 +30,7 @@ V_PLANES = (11,)
 POOL_TOKENS = (256,384,384,256)
 SHARE = {15: 128, 16: 128}
 SHARE_AT = {15: 0, 16: 0}
-WARM = (5, 1, 0)
+WARM = ()
 HEAD_V_CASTS = 1
 
 
@@ -66,19 +67,14 @@ def tile_spn_w4_kernel(tc, x_bytes, x_scale, w0_words, w0_scales, w1_words, w1_s
 
         if WARM:
             zeros = keep.tile([P, 512], BF16, name="zeros")
-            warm = keep.tile([P, 1], F32, name="warm")
             nc.vector.memset(zeros[:], 0.0)
         nc.vector.memset(w0s_raw[:].bitcast(I32), 0)
-        if WARM:
-            nc.vector.memset(warm[:], 0.0)
         nc.vector.memset(w1s[:].rearrange("p g n -> p (g n)").bitcast(I32), 0)
         make_identity(nc, ident[:])
 
         def load_x(c):
             nc.sync.dma_start(out=xb[c][:], in_=x_view[:, first[c] : first[c] + CHUNKS[c], :])
 
-        if WARM:
-            nc.scalar.activation(out=warm[:], in_=warm[:], func=RELU)
         load_x(0)
         nc.sync.dma_start(out=xs_col[:], in_=x_scale.rearrange("o (n m) -> n (o m)", m=4))
         load_x(1)
@@ -130,6 +126,9 @@ def tile_spn_w4_kernel(tc, x_bytes, x_scale, w0_words, w0_scales, w1_words, w1_s
             for jj in range(count):
                 xv[c, j0 + jj] = t[:, jj, :]
             move(out=t[:].rearrange("p j k -> p (j k)"), in_=xb[c][:, j0 : j0 + count, :].rearrange("p j k -> p (j k)").bitcast(FP8))
+
+        def scalar_cast(out, in_):
+            nc.scalar.activation(out=out, in_=in_, func=COPY)
 
         def x_transpose(c, j0, count=2):
             t = psum.tile([P, 2, count, P], F32, name="xt", tag=side_bank(), bufs=1)
@@ -257,7 +256,7 @@ def tile_spn_w4_kernel(tc, x_bytes, x_scale, w0_words, w0_scales, w1_words, w1_s
         if WARM:
             dummies(WARM[0])
         x_cast(0, 0, 1, nc.vector.tensor_copy)
-        x_cast(0, 1, 1, nc.scalar.copy)
+        x_cast(0, 1, 1, scalar_cast)
         x_transpose(0, 0, 1)
         x_transpose(0, 1, 1)
         x_cast(1, 0, 1, nc.vector.tensor_copy)

@@ -27,7 +27,7 @@ FLOPS = 2 * B * X * N + 2 * B * H * OS
 CHUNKS = (2, 4, 4, 4, 2)
 HEAD_CHUNKS = 2
 V_PLANES = (11,)
-POOL_TOKENS = (256,384,384,256)
+POOL_TOKENS = (256, 400, 400, 256)
 SHARE = {15: 128, 16: 128}
 SHARE_AT = {15: 0, 16: 0}
 WARM = ()
@@ -158,7 +158,7 @@ def tile_spn_w4_kernel(tc, x_bytes, x_scale, w0_words, w0_scales, w1_words, w1_s
             c, g = units[s]
             n = n or CHUNKS[c] * P
             if t == 0 and a == 0:
-                hp[s] = work.tile([P, 4, 512], BF16, name="hp", bufs=6, align_bytes=64)
+                hp[s] = work.tile([P, 4, 512 + 16], BF16, name="hp", bufs=6, align_bytes=64)
             z = psum.tile([P, 512], F32, name="z", bufs=5)
             m0 = 512 * g + P * t
             nc.tensor.matmul_mx(
@@ -292,9 +292,13 @@ def tile_spn_w4_kernel(tc, x_bytes, x_scale, w0_words, w0_scales, w1_words, w1_s
                 if c > 0:
                     h_quantize(u - 1, 0, tokens(u - 1))
                     whole_stage2(c - 1, 0)
-                if cut:
-                    weave(nc.vector.tensor_copy, u, 0, cut)
-                if cut < n:
+                if 0 < c < last - 1:
+                    x_cast(c + 2, 0, CHUNKS[c + 2], nc.vector.tensor_copy)
+                    hg[u, 0] = work.tile([P, 4 * n], BF16, name="hg", tag="hand", bufs=1, align_bytes=64)
+                    pool_copy(out=hg[u, 0][:, 4 * cut :].rearrange("p (n t) -> p n t", t=4), in_=hp[u][:, :, cut:n].rearrange("p t n -> p n t"))
+                else:
+                    if cut:
+                        weave(nc.vector.tensor_copy, u, 0, cut)
                     weave(pool_copy, u, cut, n, "hand", 1)
                 for j in range(0, CHUNKS[c + 1], 2):
                     x_scale_out(c + 1, j)
@@ -310,6 +314,15 @@ def tile_spn_w4_kernel(tc, x_bytes, x_scale, w0_words, w0_scales, w1_words, w1_s
                 for k in V_PLANES:
                     if k // 16 == c:
                         v_plane(k)
+                if 0 < c < last - 1:
+                    if cut:
+                        nc.vector.tensor_copy(
+                            out=hg[u, 0][:, : 4 * cut].rearrange("p (c i t) -> p c t i", t=4, i=4),
+                            in_=hp[u][:, :, :cut].rearrange("p t (c i) -> p c t i", i=4),
+                        )
+                    x_quantize(c + 1)
+                    h_quantize(u, 0, n)
+                    return
                 if cut:
                     h_quantize(u, 0, cut)
                 x_quantize(c + 1)
@@ -356,7 +369,7 @@ def tile_spn_w4_kernel(tc, x_bytes, x_scale, w0_words, w0_scales, w1_words, w1_s
                 finish(last - 1, 0)
             if u == 1 and 1:
                 x_cast(2, 4 - 1, 1, nc.vector.tensor_copy)
-            if g == G - 1 and c + 3 < n_chunks:
+            if g == G - 1 and c + 3 < n_chunks and False:
                 x_cast(c + 3, 0, CHUNKS[c + 3], nc.vector.tensor_copy)
 
         n_planes = 4 * n_units

@@ -21,33 +21,39 @@ MAX = mybir.AluOpType.max
 P = 128
 B, X, N, OS = 2048, 512, 2304, 256
 H = N - OS
-G = H // 512
+PASS = 512
+G = H // PASS
+T = 4
 FLOPS = 2 * B * X * N + 2 * B * H * OS
 
 CHUNKS = (2, 4, 4, 4, 2)
-HEAD_CHUNKS = 2
-V_PLANES = (11,)
-POOL_TOKENS = (256, 400, 400, 256)
-SHARE = {15: 128, 16: 128}
-SHARE_AT = {15: 0, 16: 0}
-WARM = ()
-HEAD_V_CASTS = 1
+MAX_TOKENS = max(CHUNKS) * P
+PLANE_BANKS = 5
+SIDE_BANKS = 3
+POOL_TOKENS = (256, 448, 448, 256)
+SCALAR_TOKENS = (128, 64)
+VECTOR_PLANE = 2 * T + 3
+PLANE_PAD = 16
 
 
 def tile_spn_w4_kernel(tc, x_bytes, x_scale, w0_words, w0_scales, w1_words, w1_scales, biases, out):
     nc = tc.nc
     n_chunks = len(CHUNKS)
     last = n_chunks - 1
-    first = [sum(CHUNKS[:c]) for c in range(n_chunks)]
-    units = [(c, g) for c in range(n_chunks) for g in range(G)]
-    n_units = len(units)
+    first_tile = [sum(CHUNKS[:c]) for c in range(n_chunks)]
+    n_units = n_chunks * G
+    last_start = last * G
+    scalar_tokens = dict(zip((last_start - 1, last_start), SCALAR_TOKENS))
     x_view = x_bytes.rearrange("(p j) k -> p j k", j=B // P)
     out_view = out.rearrange("(p j) n -> p j n", j=B // P)
+
+    def tokens(u):
+        return CHUNKS[u // G] * P
 
     with ExitStack() as ctx:
         keep = ctx.enter_context(tc.tile_pool(name="keep", bufs=1))
         work = ctx.enter_context(tc.tile_pool(name="work", bufs=4))
-        psum = ctx.enter_context(tc.psum_pool(name="psum", bufs=5))
+        psum = ctx.enter_context(tc.psum_pool(name="psum", bufs=PLANE_BANKS))
         ctx.enter_context(tc.manual_schedule())
 
         ident = keep.tile([P, P], F32, name="ident")
@@ -57,38 +63,37 @@ def tile_spn_w4_kernel(tc, x_bytes, x_scale, w0_words, w0_scales, w1_words, w1_s
         w0s_perm = keep.tile([P, H], U8, name="w0s_perm", align_bytes=64)
         w1 = keep.tile([P, G, 2 * OS], U8, name="w1", align_bytes=64)
         w1s = keep.tile([P, G, OS], U8, name="w1s", align_bytes=64)
-        bias_h = keep.tile([P, G, 4], BF16, name="bias_h")
+        bias_h = keep.tile([P, G, T], BF16, name="bias_h")
         bias_o = keep.tile([P, OS], BF16, name="bias_o")
-        xs_col = keep.tile([P, 4], F32, name="xs_col")
-        xb = []
+        xs_col = keep.tile([P, T], F32, name="xs_col")
+        x_raw = []
         for c in range(n_chunks):
-            xb_c = keep.tile([P, CHUNKS[c], X], U8, name="xbytes%d" % c, align_bytes=64)
-            xb.append(xb_c)
+            raw = keep.tile([P, CHUNKS[c], X], U8, name="xbytes%d" % c, align_bytes=64)
+            x_raw.append(raw)
 
-        if WARM:
-            zeros = keep.tile([P, 512], BF16, name="zeros")
-            nc.vector.memset(zeros[:], 0.0)
         nc.vector.memset(w0s_raw[:].bitcast(I32), 0)
         nc.vector.memset(w1s[:].rearrange("p g n -> p (g n)").bitcast(I32), 0)
         make_identity(nc, ident[:])
 
         def load_x(c):
-            nc.sync.dma_start(out=xb[c][:], in_=x_view[:, first[c] : first[c] + CHUNKS[c], :])
+            nc.sync.dma_start(out=x_raw[c][:], in_=x_view[:, first_tile[c] : first_tile[c] + CHUNKS[c], :])
+
+        def load_w0(n0, n1):
+            nc.sync.dma_start(out=w0_raw[:, 2 * n0 : 2 * n1], in_=w0_words[0, :, 2 * n0 : 2 * n1])
 
         load_x(0)
-        nc.sync.dma_start(out=xs_col[:], in_=x_scale.rearrange("o (n m) -> n (o m)", m=4))
+        nc.sync.dma_start(out=xs_col[:], in_=x_scale.rearrange("o (p t) -> p (o t)", t=T))
         load_x(1)
-        nc.sync.dma_start(out=w0_raw[:, 0:1024], in_=w0_words[0, :, 0:1024])
+        load_w0(0, PASS)
         for q in range(4):
             nc.sync.dma_start(
                 out=w0s_raw[32 * q : 32 * q + 4, :].bitcast(I32),
                 in_=w0_scales[0, 4 * q : 4 * q + 4, :].bitcast(I32),
             )
         load_x(2)
-        nc.sync.dma_start(out=bias_h[:], in_=biases[0:H].rearrange("(g p t) -> p g t", g=G, p=P, t=4))
-        nc.sync.dma_start(out=w0_raw[:, 1024:2048], in_=w0_words[0, :, 1024:2048])
-        pass
-        nc.sync.dma_start(out=w0_raw[:, 2048:4608], in_=w0_words[0, :, 2048:4608])
+        nc.sync.dma_start(out=bias_h[:], in_=biases[0:H].rearrange("(g p t) -> p g t", g=G, p=P, t=T))
+        load_w0(PASS, 2 * PASS)
+        load_w0(2 * PASS, N)
         nc.sync.dma_start(out=w1[:], in_=w1_words.rearrange("g p n -> p g n"))
         for q in range(4):
             nc.sync.dma_start(
@@ -99,301 +104,288 @@ def tile_spn_w4_kernel(tc, x_bytes, x_scale, w0_words, w0_scales, w1_words, w1_s
             load_x(c)
         nc.sync.dma_start(out=bias_o[:], in_=biases[H:N].partition_broadcast(P))
 
-        xv, xt, xg, xq, xqs = {}, {}, {}, {}, {}
-        held = {}
-        hp, hg, hq, hqs, acc = {}, {}, {}, {}, {}
-
-        taken = []
+        x_wide, x_turned, x_woven, x_codes, x_scales = {}, {}, {}, {}, {}
+        z_kept, h_planes, h_woven, h_codes, h_scales, sums = {}, {}, {}, {}, {}, {}
+        side_turns = []
 
         def side_bank():
-            taken.append(len(taken) % 3)
-            return "side%d" % taken[-1]
+            side_turns.append(len(side_turns) % SIDE_BANKS)
+            return "side%d" % side_turns[-1]
 
-        def permute_codes(g0, g1):
+
+        def permute_words(g0, g1):
+            cols = slice(2 * PASS * g0, 2 * PASS * g1)
             nc.vector.tensor_copy(
-                out=w0_perm[:, 1024 * g0 : 1024 * g1].bitcast(U16).rearrange("p (g t m) -> p g t m", t=4, m=P),
-                in_=w0_raw[:, 1024 * g0 : 1024 * g1].bitcast(U16).rearrange("p (g m t) -> p g t m", t=4, m=P),
+                out=w0_perm[:, cols].bitcast(U16).rearrange("p (g t m) -> p g t m", t=T, m=P),
+                in_=w0_raw[:, cols].bitcast(U16).rearrange("p (g m t) -> p g t m", t=T, m=P),
             )
 
         def permute_scales(g0, g1):
+            cols = slice(PASS * g0, PASS * g1)
             nc.vector.tensor_copy(
-                out=w0s_perm[:, 512 * g0 : 512 * g1].rearrange("p (g t m) -> p g t m", t=4, m=P),
-                in_=w0s_raw[:, 512 * g0 : 512 * g1].rearrange("p (g m t) -> p g t m", t=4, m=P),
+                out=w0s_perm[:, cols].rearrange("p (g t m) -> p g t m", t=T, m=P),
+                in_=w0s_raw[:, cols].rearrange("p (g m t) -> p g t m", t=T, m=P),
             )
 
-        def x_cast(c, j0, count, move):
-            t = work.tile([P, count, X], BF16, name="xv", tag="xv%d" % count, bufs=8 // count, align_bytes=64)
-            for jj in range(count):
-                xv[c, j0 + jj] = t[:, jj, :]
-            move(out=t[:].rearrange("p j k -> p (j k)"), in_=xb[c][:, j0 : j0 + count, :].rearrange("p j k -> p (j k)").bitcast(FP8))
 
-        def scalar_cast(out, in_):
+        def x_cast(c, j0, count, cast):
+            wide = work.tile([P, count, X], BF16, name="xv", tag="xv%d" % count, bufs=8 // count, align_bytes=64)
+            for jj in range(count):
+                x_wide[c, j0 + jj] = wide[:, jj, :]
+            cast(
+                out=wide[:].rearrange("p j k -> p (j k)"),
+                in_=x_raw[c][:, j0 : j0 + count, :].rearrange("p j k -> p (j k)").bitcast(FP8),
+            )
+
+        def scalar_activation_cast(out, in_):
             nc.scalar.activation(out=out, in_=in_, func=COPY)
 
-        def x_transpose(c, j0, count=2):
-            t = psum.tile([P, 2, count, P], F32, name="xt", tag=side_bank(), bufs=1)
-            xt[c, j0] = t
+        def x_transpose(c, j0, count):
+            bank = psum.tile([P, 2, count, P], F32, name="xt", tag=side_bank(), bufs=1)
+            x_turned[c, j0] = bank
             for jj in range(count):
-                words = xv[c, j0 + jj].bitcast(F32)
+                words = x_wide[c, j0 + jj].bitcast(F32)
                 for u in range(2):
-                    nc.tensor.transpose(t[:, u, jj, :], words[:, u : X // 2 : 2], ident[:])
+                    nc.tensor.transpose(bank[:, u, jj, :], words[:, u : X // 2 : 2], ident[:])
 
-        def x_scale_out(c, j0, count=2):
+        def x_scale_out(c, j0, count):
             if j0 == 0:
-                xg[c] = work.tile([P, 2048], BF16, name="xg", bufs=2, align_bytes=64)
+                x_woven[c] = work.tile([P, T * MAX_TOKENS], BF16, name="xg", bufs=2, align_bytes=64)
+            halves = x_turned[c, j0][:].rearrange("p u j r -> p (u j r)").bitcast(BF16)
             nc.vector.tensor_tensor(
-                out=xg[c][:, 512 * j0 : 512 * (j0 + count)].rearrange("p (r u e) -> p r u e", u=2, e=2),
-                in0=xt[c, j0][:].rearrange("p u j r -> p (u j r)").bitcast(BF16).rearrange("p (u r e) -> p r u e", u=2, e=2),
+                out=x_woven[c][:, T * P * j0 : T * P * (j0 + count)].rearrange("p (r u e) -> p r u e", u=2, e=2),
+                in0=halves.rearrange("p (u r e) -> p r u e", u=2, e=2),
                 in1=xs_col[:].rearrange("p (o u e) -> p o u e", o=1, u=2).to_broadcast([P, count * P, 2, 2]),
                 op=MULT,
             )
 
         def x_quantize(c):
             n = CHUNKS[c] * P
-            xq[c] = work.tile([P, 512], U32, name="xq", bufs=n_chunks, align_bytes=64)
-            xqs[c] = work.tile([P, 512], U8, name="xqs", bufs=n_chunks, align_bytes=64)
-            nc.vector.quantize_mx(out=xq[c][:, :n].bitcast(FP8X4), scales=xqs[c][:, :n], in_=xg[c][:, : 4 * n])
+            x_codes[c] = work.tile([P, MAX_TOKENS], U32, name="xq", bufs=n_chunks, align_bytes=64)
+            x_scales[c] = work.tile([P, MAX_TOKENS], U8, name="xqs", bufs=n_chunks, align_bytes=64)
+            nc.vector.quantize_mx(out=x_codes[c][:, :n].bitcast(FP8X4), scales=x_scales[c][:, :n], in_=x_woven[c][:, : T * n])
 
-        def plane(s, t, a=0, n=None):
-            c, g = units[s]
-            n = n or CHUNKS[c] * P
-            if t == 0 and a == 0:
-                hp[s] = work.tile([P, 4, 512 + 16], BF16, name="hp", bufs=6, align_bytes=64)
-            z = psum.tile([P, 512], F32, name="z", bufs=5)
-            m0 = 512 * g + P * t
+
+        def plane(k):
+            u, t = divmod(k, T)
+            c, g = divmod(u, G)
+            n = tokens(u)
+            if t == 0:
+                h_planes[u] = work.tile([P, T, MAX_TOKENS + PLANE_PAD], BF16, name="hp", bufs=6, align_bytes=64)
+            z = psum.tile([P, MAX_TOKENS], F32, name="z", bufs=PLANE_BANKS)
+            m0 = PASS * g + P * t
             nc.tensor.matmul_mx(
                 out=z[:, :n],
                 lhsT=w0_perm[:, 2 * m0 : 2 * (m0 + P)].bitcast(FP4X4),
                 lhsT_scale=w0s_perm[:, m0 : m0 + P],
-                rhs=xq[c][:, a : a + n].bitcast(FP8X4),
-                rhs_scale=xqs[c][:, a : a + n],
+                rhs=x_codes[c][:, :n].bitcast(FP8X4),
+                rhs_scale=x_scales[c][:, :n],
                 start=True,
                 stop=True,
             )
-            if 4 * s + t in V_PLANES:
-                held[4 * s + t] = z
+            if k == VECTOR_PLANE:
+                z_kept[k] = z
             else:
-                nc.scalar.activation(out=hp[s][:, t, a : a + n], in_=z[:, :n], func=RELU, bias=bias_h[:, g, t : t + 1])
+                nc.scalar.activation(out=h_planes[u][:, t, :n], in_=z[:, :n], func=RELU, bias=bias_h[:, g, t : t + 1])
 
-        def v_plane(k):
-            s, t = divmod(k, 4)
-            c, g = units[s]
-            n = CHUNKS[c] * P
-            nc.vector.tensor_scalar(out=hp[s][:, t, :n], in0=held[k][:, :n], scalar1=bias_h[:, g, t : t + 1], scalar2=0.0, op0=ADD, op1=MAX)
-
-        def pool_copy(out, in_):
-            nc.gpsimd.tensor_scalar(out=out, in0=in_, scalar1=1.0, scalar2=0.0, op0=MULT, op1=ADD)
-
-        def weave(move, s, a, b, tag="hg", bufs=4):
-            if (s, a) not in hg:
-                hg[s, a] = work.tile([P, 4 * (b - a)], BF16, name="hg", tag=tag, bufs=bufs, align_bytes=64)
-            if move is pool_copy:
-                move(out=hg[s, a][:].rearrange("p (n t) -> p n t", t=4), in_=hp[s][:, :, a:b].rearrange("p t n -> p n t"))
-            else:
-                e = b - SHARE.get(s, 0) * (b == tokens(s))
-                move(
-                    out=hg[s, a][:, : 4 * (e - a)].rearrange("p (c i t) -> p c t i", t=4, i=4),
-                    in_=hp[s][:, :, a:e].rearrange("p t (c i) -> p c t i", i=4),
-                )
-
-        def scalar_share(s, a):
-            b = tokens(s)
-            e = b - SHARE[s]
-            hg[s, a] = work.tile([P, 4 * (b - a)], BF16, name="hg", tag="hs", bufs=3, align_bytes=64)
-            nc.scalar.copy(
-                out=hg[s, a][:, 4 * (e - a) :].rearrange("p (c i t) -> p c t i", t=4, i=4),
-                in_=hp[s][:, :, e:b].rearrange("p t (c i) -> p c t i", i=4),
+        def vector_plane_out(k):
+            u, t = divmod(k, T)
+            n = tokens(u)
+            nc.vector.tensor_scalar(
+                out=h_planes[u][:, t, :n], in0=z_kept[k][:, :n], scalar1=bias_h[:, u % G, t : t + 1], scalar2=0.0, op0=ADD, op1=MAX
             )
 
-        def h_quantize(s, a, b):
-            if s not in hq:
-                hq[s] = work.tile([P, 512], U32, name="hq", bufs=12, align_bytes=64)
-                hqs[s] = work.tile([P, 512], U8, name="hqs", bufs=12, align_bytes=64)
-            nc.vector.quantize_mx(out=hq[s][:, a:b].bitcast(FP8X4), scales=hqs[s][:, a:b], in_=hg[s, a][:])
+        def woven_tile(u, a, b, tag, bufs):
+            h_woven[u, a] = work.tile([P, T * (b - a)], BF16, name="hg", tag=tag, bufs=bufs, align_bytes=64)
 
-        def out_pass(dst, lhs, lhs_scales, j, rhs, rhs_scales, start, stop):
+        def weave(copy, u, a, lo, hi):
+            copy(
+                out=h_woven[u, a][:, T * (lo - a) : T * (hi - a)].rearrange("p (c i t) -> p c t i", t=T, i=4),
+                in_=h_planes[u][:, :, lo:hi].rearrange("p t (c i) -> p c t i", i=4),
+            )
+
+        def weave_own(copy, u, a, b):
+            woven_tile(u, a, b, "hg", 4)
+            weave(copy, u, a, a, b)
+
+        def pool_weave(u, a, lo, hi):
+            nc.gpsimd.tensor_scalar(
+                out=h_woven[u, a][:, T * (lo - a) : T * (hi - a)].rearrange("p (n t) -> p n t", t=T),
+                in0=h_planes[u][:, :, lo:hi].rearrange("p t n -> p n t"),
+                scalar1=1.0,
+                scalar2=0.0,
+                op0=MULT,
+                op1=ADD,
+            )
+
+        def h_quantize(u, a, b):
+            if u not in h_codes:
+                h_codes[u] = work.tile([P, MAX_TOKENS], U32, name="hq", bufs=3 * G, align_bytes=64)
+                h_scales[u] = work.tile([P, MAX_TOKENS], U8, name="hqs", bufs=3 * G, align_bytes=64)
+            nc.vector.quantize_mx(out=h_codes[u][:, a:b].bitcast(FP8X4), scales=h_scales[u][:, a:b], in_=h_woven[u, a][:])
+
+
+        def out_pass(dst, codes, scales, j, w, w_scales, start, stop):
             cols = slice(j * P, (j + 1) * P)
             nc.tensor.matmul_mx(
                 out=dst,
-                lhsT=lhs[:, cols].bitcast(FP8X4),
-                lhsT_scale=lhs_scales[:, cols],
-                rhs=rhs.bitcast(FP4X4),
-                rhs_scale=rhs_scales,
+                lhsT=codes[:, cols].bitcast(FP8X4),
+                lhsT_scale=scales[:, cols],
+                rhs=w.bitcast(FP4X4),
+                rhs_scale=w_scales,
                 start=start,
                 stop=stop,
             )
 
-        def stage2(s, tiles):
-            c, g = units[s]
+        def unit_passes(u, tiles):
+            c, g = divmod(u, G)
             per_bank = 1 if c == last else 2
             for j in tiles:
+                bank, place = divmod(j, per_bank)
                 if g == 0:
-                    if j % per_bank == 0:
-                        tag, bufs = (side_bank(), 1) if c < last or j == 0 else ("z", 5)
-                        acc[c, j // per_bank] = psum.tile([P, per_bank, OS], F32, name="o", tag=tag, bufs=bufs)
-                    out_pass(acc[c, j // per_bank][:, j % per_bank, :], xq[c], xqs[c], j, w0_raw[:, 2 * H : 2 * N], w0s_raw[:, H:N], j % per_bank == 0, False)
-                closes = g == G - 1 and j % per_bank == per_bank - 1
-                out_pass(acc[c, j // per_bank][:, j % per_bank, :], hq[s], hqs[s], j, w1[:, g, :], w1s[:, g, :], False, closes)
+                    if place == 0:
+                        tag, bufs = ("z", PLANE_BANKS) if c == last and j > 0 else (side_bank(), 1)
+                        sums[c, bank] = psum.tile([P, per_bank, OS], F32, name="o", tag=tag, bufs=bufs)
+                    w_out, w_out_scales = w0_raw[:, 2 * H : 2 * N], w0s_raw[:, H:N]
+                    out_pass(sums[c, bank][:, place, :], x_codes[c], x_scales[c], j, w_out, w_out_scales, place == 0, False)
+                closes = g == G - 1 and place == per_bank - 1
+                out_pass(sums[c, bank][:, place, :], h_codes[u], h_scales[u], j, w1[:, g, :], w1s[:, g, :], False, closes)
 
-        def finish(c, pair):
+        def pair_passes(c, pair):
+            for g in range(G):
+                unit_passes(G * c + g, (2 * pair, 2 * pair + 1))
+
+        def store_pair(c, pair):
             res = work.tile([P, 2, OS], F32, name="res", bufs=4)
-            nc.vector.tensor_tensor(out=res[:], in0=acc[c, pair][:], in1=bias_o[:].unsqueeze(1).to_broadcast([P, 2, OS]), op=ADD)
-            j0 = first[c] + 2 * pair
+            nc.vector.tensor_tensor(out=res[:], in0=sums[c, pair][:], in1=bias_o[:].unsqueeze(1).to_broadcast([P, 2, OS]), op=ADD)
+            j0 = first_tile[c] + 2 * pair
             nc.sync.dma_start(out=out_view[:, j0 : j0 + 2, :], in_=res[:])
 
-        def finish_last(j):
+        def store_last(j):
             res = work.tile([P, OS], F32, name="tail_res", bufs=2)
-            nc.vector.tensor_tensor(out=res[:], in0=acc[last, j][:, 0, :], in1=bias_o[:], op=ADD)
-            nc.sync.dma_start(out=out_view[:, first[last] + j, :], in_=res[:])
+            nc.vector.tensor_tensor(out=res[:], in0=sums[last, j][:, 0, :], in1=bias_o[:], op=ADD)
+            nc.sync.dma_start(out=out_view[:, first_tile[last] + j, :], in_=res[:])
 
-        def dummies(k):
-            if not k:
-                return
-            d = psum.tile([P, 512], F32, name="z", bufs=5)
-            for i in range(k):
-                nc.tensor.matmul(d[:], lhsT=zeros[:, :P], rhs=zeros[:], start=True, stop=True)
-
-        if WARM:
-            dummies(WARM[0])
         x_cast(0, 0, 1, nc.vector.tensor_copy)
-        x_cast(0, 1, 1, scalar_cast)
+        x_cast(0, 1, 1, scalar_activation_cast)
         x_transpose(0, 0, 1)
         x_transpose(0, 1, 1)
         x_cast(1, 0, 1, nc.vector.tensor_copy)
         for j in range(1, CHUNKS[1]):
             x_cast(1, j, 1, nc.scalar.copy)
-        permute_codes(0, 1)
-        x_transpose(1, 0)
-        if WARM:
-            dummies(WARM[1])
+        permute_words(0, 1)
+        x_transpose(1, 0, 2)
         for j in range(CHUNKS[0]):
             x_scale_out(0, j, 1)
-        x_transpose(1, 2)
+        x_transpose(1, 2, 2)
         x_cast(2, 0, 2, nc.scalar.copy)
         permute_scales(0, 1)
         x_quantize(0)
         permute_scales(1, 2)
-        permute_codes(1, 2)
+        permute_words(1, 2)
         permute_scales(2, G)
-        permute_codes(2, G)
+        permute_words(2, G)
 
-        def tokens(u):
-            return CHUNKS[units[u][0]] * P
 
-        def whole_stage2(c, pair):
-            for g in range(G):
-                stage2(G * c + g, (2 * pair, 2 * pair + 1))
-
-        def vector_step(u):
-            c, g = units[u]
+        def window_open(c):
+            u = G * c
             n = tokens(u)
-            if g == 0 and c < last:
-                cut = n - POOL_TOKENS[c]
-                if c > 0:
-                    h_quantize(u - 1, 0, tokens(u - 1))
-                    whole_stage2(c - 1, 0)
-                if 0 < c < last - 1:
-                    x_cast(c + 2, 0, CHUNKS[c + 2], nc.vector.tensor_copy)
-                    hg[u, 0] = work.tile([P, 4 * n], BF16, name="hg", tag="hand", bufs=1, align_bytes=64)
-                    pool_copy(out=hg[u, 0][:, 4 * cut :].rearrange("p (n t) -> p n t", t=4), in_=hp[u][:, :, cut:n].rearrange("p t n -> p n t"))
-                else:
-                    if cut:
-                        weave(nc.vector.tensor_copy, u, 0, cut)
-                    weave(pool_copy, u, cut, n, "hand", 1)
-                for j in range(0, CHUNKS[c + 1], 2):
-                    x_scale_out(c + 1, j)
-                if c > 0:
-                    finish(c - 1, 0)
-                return
-            rest_of_step(u)
+            cut = n - POOL_TOKENS[c]
+            if c > 0:
+                h_quantize(u - 1, 0, tokens(u - 1))
+                pair_passes(c - 1, 0)
+            if 0 < c < last - 1:
+                x_cast(c + 2, 0, CHUNKS[c + 2], nc.vector.tensor_copy)
+                woven_tile(u, 0, n, "hand", 1)
+                pool_weave(u, 0, cut, n)
+            else:
+                if cut:
+                    weave_own(nc.vector.tensor_copy, u, 0, cut)
+                woven_tile(u, cut, n, "hand", 1)
+                pool_weave(u, cut, cut, n)
+            for j in range(0, CHUNKS[c + 1], 2):
+                x_scale_out(c + 1, j, 2)
+            if c > 0:
+                store_pair(c - 1, 0)
 
-        def window_end(u):
-                c, g = units[u]
-                n = tokens(u)
-                cut = n - POOL_TOKENS[c]
-                for k in V_PLANES:
-                    if k // 16 == c:
-                        v_plane(k)
-                if 0 < c < last - 1:
-                    if cut:
-                        nc.vector.tensor_copy(
-                            out=hg[u, 0][:, : 4 * cut].rearrange("p (c i t) -> p c t i", t=4, i=4),
-                            in_=hp[u][:, :, :cut].rearrange("p t (c i) -> p c t i", i=4),
-                        )
-                    x_quantize(c + 1)
-                    h_quantize(u, 0, n)
-                    return
+        def window_close(c):
+            u = G * c
+            n = tokens(u)
+            cut = n - POOL_TOKENS[c]
+            if c == 0:
+                vector_plane_out(VECTOR_PLANE)
+            if 0 < c < last - 1:
+                weave(nc.vector.tensor_copy, u, 0, 0, cut)
+                x_quantize(c + 1)
+                h_quantize(u, 0, n)
+            else:
                 if cut:
                     h_quantize(u, 0, cut)
                 x_quantize(c + 1)
-                if cut < n:
-                    h_quantize(u, cut, n)
+                h_quantize(u, cut, n)
 
-        def rest_of_step(u):
-            c, g = units[u]
+        def plain_step(u):
+            c, g = divmod(u, G)
             n = tokens(u)
-            if u == n_units - 1:
-                def wa():
-                    weave(nc.vector.tensor_copy, u, 0, P)
-                def wb():
-                    weave(nc.scalar.copy, u, P, n)
-                def qp():
-                    h_quantize(u - 1, 0, tokens(u - 1))
-                    stage2(u - 1, range(CHUNKS[last]))
-                def qa():
-                    h_quantize(u, 0, P)
-                    stage2(u, (0,))
-                def qb():
-                    h_quantize(u, P, n)
-                    stage2(u, (1,))
-                def f3():
-                    finish(last - 1, 1)
-                def fa():
-                    finish_last(0)
-                def fb():
-                    finish_last(1)
-                for f in (wa, wb, qp, qa, qb, f3, fa, fb):
-                    f()
-                return
             if g == G - 1 and c + 1 < last:
-                weave(nc.vector.tensor_copy, u, 0, n, "hand", 1)
-            elif (u, 0) not in hg or u in SHARE:
-                weave(nc.vector.tensor_copy, u, 0, n)
-            if (g > 1 or c == last) and u != G * last:
+                woven_tile(u, 0, n, "hand", 1)
+                weave(nc.vector.tensor_copy, u, 0, 0, n)
+            elif u in scalar_tokens:
+                weave(nc.vector.tensor_copy, u, 0, 0, n - scalar_tokens[u])
+            else:
+                weave_own(nc.vector.tensor_copy, u, 0, n)
+            if g > 1 or u > last_start:
                 h_quantize(u - 1, 0, tokens(u - 1))
-            if u == G * last - 1:
+            if u == last_start - 1:
                 h_quantize(u, 0, n)
-            if g == 3 and 0 < c < last and CHUNKS[c - 1] > 2:
-                finish(c - 1, 1)
-            if u == G * last + 1:
-                finish(last - 1, 0)
-            if u == 1 and 1:
-                x_cast(2, 4 - 1, 1, nc.vector.tensor_copy)
-            if g == G - 1 and c + 3 < n_chunks and False:
-                x_cast(c + 3, 0, CHUNKS[c + 3], nc.vector.tensor_copy)
+            if g == G - 1 and 0 < c < last and CHUNKS[c - 1] > 2:
+                store_pair(c - 1, 1)
+            if u == last_start + 1:
+                store_pair(last - 1, 0)
+            if u == 1:
+                x_cast(2, 3, 1, nc.vector.tensor_copy)
 
-        n_planes = 4 * n_units
-        for k in range(n_planes + 4 + 2):
-            s, t = divmod(k, 4)
-            c, g = divmod(s, G)
-            if k < n_planes - 4 * 0:
-                plane(s, t)
-            elif k < n_planes:
-                plane(s, 2 * t % 4, t // 2 * P, P)
-                plane(s, 2 * t % 4 + 1, t // 2 * P, P)
-            if t == 0 and s - 1 in SHARE:
-                scalar_share(s - 1, SHARE_AT[s - 1])
-            if k == 14 and 1 < 2:
-                x_cast(2, 2, 2 - 1, nc.scalar.copy)
-            if k % 16 == 2 and HEAD_CHUNKS <= c + 1 < n_chunks:
-                for pair in range(CHUNKS[c + 1] // 2):
-                    x_transpose(c + 1, 2 * pair)
-            if k % 16 == 13 and 0 < c < last and CHUNKS[c - 1] > 2:
-                whole_stage2(c - 1, 1)
-            for u in range(G * (last - 1), n_units - 2):
-                if k == min(max(4 * u + 17, 4 * G * (last - 1) + 17), n_planes + 2):
-                    stage2(u, range(CHUNKS[units[u][0]]))
-            if k >= 7 + 2 and (k - 2) % 4 == 3:
-                vector_step((k - 2) // 4 - 1)
-            if k // 16 < last and k % 16 == max([7 + 2] + [v % 16 for v in V_PLANES if v // 16 == k // 16]):
-                window_end(k // 16 * G)
+        def last_step(u):
+            weave_own(nc.vector.tensor_copy, u, 0, P)
+            weave_own(nc.scalar.copy, u, P, 2 * P)
+            h_quantize(u - 1, 0, tokens(u - 1))
+            unit_passes(u - 1, range(CHUNKS[last]))
+            for j in range(CHUNKS[last]):
+                h_quantize(u, j * P, (j + 1) * P)
+                unit_passes(u, (j,))
+            store_pair(last - 1, 1)
+            for j in range(CHUNKS[last]):
+                store_last(j)
+
+        def step_plane(u):
+            return T * (u + 1) + PLANE_BANKS
+
+        n_planes = T * n_units
+        for k in range(step_plane(n_units - 1) + 1):
+            c, place = divmod(k, T * G)
+            if k < n_planes:
+                plane(k)
+            for u in scalar_tokens:
+                if k == T * (u + 1):
+                    woven_tile(u, 0, tokens(u), "hs", 3)
+                    weave(nc.scalar.copy, u, 0, tokens(u) - scalar_tokens[u], tokens(u))
+            if k == T * G - 2:
+                x_cast(2, 2, 1, nc.scalar.copy)
+            if place == 2 and 0 < c < last:
+                for j in range(0, CHUNKS[c + 1], 2):
+                    x_transpose(c + 1, j, 2)
+            if k == step_plane(G * c + 1) and 0 < c < last and CHUNKS[c - 1] > 2:
+                pair_passes(c - 1, 1)
+            for u in range(last_start - G, n_units - 2):
+                if k == min(step_plane(u + 2), step_plane(n_units - 2) + 1):
+                    unit_passes(u, range(CHUNKS[u // G]))
+            for u in range(n_units):
+                if k == step_plane(u):
+                    if u == n_units - 1:
+                        last_step(u)
+                    elif u % G == 0 and u < last_start:
+                        window_open(u // G)
+                    else:
+                        plain_step(u)
+            if c < last and k == (VECTOR_PLANE if c == 0 else step_plane(G * c)):
+                window_close(c)

@@ -92,6 +92,7 @@ def tile_spn_w4_kernel(tc, x_bytes, x_scale, w0_words, w0_scales, w1_words, w1_s
             )
         load_x(2)
         nc.sync.dma_start(out=bias_h[:], in_=biases[0:H].rearrange("(g p t) -> p g t", g=G, p=P, t=T))
+        load_x(3)
         load_w0(PASS, 2 * PASS)
         load_w0(2 * PASS, N)
         nc.sync.dma_start(out=w1[:], in_=w1_words.rearrange("g p n -> p g n"))
@@ -100,8 +101,7 @@ def tile_spn_w4_kernel(tc, x_bytes, x_scale, w0_words, w0_scales, w1_words, w1_s
                 out=w1s[32 * q : 32 * q + 4].bitcast(I32),
                 in_=w1_scales[:, 4 * q : 4 * q + 4, :].rearrange("g r n -> r g n").bitcast(I32),
             )
-        for c in range(3, n_chunks):
-            load_x(c)
+        load_x(last)
         nc.sync.dma_start(out=bias_o[:], in_=biases[H:N].partition_broadcast(P))
 
         x_wide, x_turned, x_woven, x_codes, x_scales = {}, {}, {}, {}, {}
@@ -129,7 +129,7 @@ def tile_spn_w4_kernel(tc, x_bytes, x_scale, w0_words, w0_scales, w1_words, w1_s
 
 
         def x_cast(c, j0, count, cast):
-            wide = work.tile([P, count, X], BF16, name="xv", tag="xv%d" % count, bufs=8 // count, align_bytes=64)
+            wide = keep.tile([P, count, X], BF16, name="xv%d_%d" % (c, j0), align_bytes=64)
             for jj in range(count):
                 x_wide[c, j0 + jj] = wide[:, jj, :]
             cast(
@@ -279,6 +279,8 @@ def tile_spn_w4_kernel(tc, x_bytes, x_scale, w0_words, w0_scales, w1_words, w1_s
             x_scale_out(0, j, 1)
         x_transpose(1, 2, 2)
         x_cast(2, 0, 2, nc.scalar.copy)
+        x_cast(2, 2, 2, nc.scalar.copy)
+        x_cast(3, 0, 2, nc.scalar.copy)
         permute_scales(0, 1)
         x_quantize(0)
         permute_scales(1, 2)
@@ -295,7 +297,7 @@ def tile_spn_w4_kernel(tc, x_bytes, x_scale, w0_words, w0_scales, w1_words, w1_s
                 h_quantize(u - 1, 0, tokens(u - 1))
                 pair_passes(c - 1, 0)
             if 0 < c < last - 1:
-                x_cast(c + 2, 0, CHUNKS[c + 2], nc.vector.tensor_copy)
+                x_cast(c + 2, CHUNKS[c + 2] - 2, 2, nc.vector.tensor_copy)
                 woven_tile(u, 0, n, "hand", 1)
                 pool_weave(u, 0, cut, n)
             else:
@@ -342,8 +344,6 @@ def tile_spn_w4_kernel(tc, x_bytes, x_scale, w0_words, w0_scales, w1_words, w1_s
                 store_pair(c - 1, 1)
             if u == last_start + 1:
                 store_pair(last - 1, 0)
-            if u == 1:
-                x_cast(2, 3, 1, nc.vector.tensor_copy)
 
         def last_step(u):
             weave_own(nc.vector.tensor_copy, u, 0, P)
@@ -369,8 +369,6 @@ def tile_spn_w4_kernel(tc, x_bytes, x_scale, w0_words, w0_scales, w1_words, w1_s
                 if k == T * (u + 1):
                     woven_tile(u, 0, tokens(u), "hs", 3)
                     weave(nc.scalar.copy, u, 0, tokens(u) - scalar_tokens[u], tokens(u))
-            if k == T * G - 2:
-                x_cast(2, 2, 1, nc.scalar.copy)
             if place == 2 and 0 < c < last:
                 for j in range(0, CHUNKS[c + 1], 2):
                     x_transpose(c + 1, j, 2)

@@ -28,12 +28,11 @@ FLOPS = 2 * B * X * N + 2 * B * H * OS
 
 CHUNKS = (2, 4, 4, 4, 2)
 MAX_TOKENS = max(CHUNKS) * P
-PLANE_BANKS = 5
-SIDE_BANKS = 3
-POOL_TOKENS = (256, 448, 448, 256)
-SCALAR_TOKENS = (128, 64)
-VECTOR_PLANE = 2 * T + 3
+PLANE_BANKS = 4
+POOL_TOKENS = (256, 480, 512, 384, 96)
+LAG = (0, 0, 0, 0, 0)
 PLANE_PAD = 16
+VECTOR_BANKS = ((2, 0),)
 
 
 def tile_spn_w4_kernel(tc, x_bytes, x_scale, w0_words, w0_scales, w1_words, w1_scales, biases, out):
@@ -42,8 +41,6 @@ def tile_spn_w4_kernel(tc, x_bytes, x_scale, w0_words, w0_scales, w1_words, w1_s
     last = n_chunks - 1
     first_tile = [sum(CHUNKS[:c]) for c in range(n_chunks)]
     n_units = n_chunks * G
-    last_start = last * G
-    scalar_tokens = dict(zip((last_start - 1, last_start), SCALAR_TOKENS))
     x_view = x_bytes.rearrange("(p j) k -> p j k", j=B // P)
     out_view = out.rearrange("(p j) n -> p j n", j=B // P)
 
@@ -58,9 +55,11 @@ def tile_spn_w4_kernel(tc, x_bytes, x_scale, w0_words, w0_scales, w1_words, w1_s
 
         ident = keep.tile([P, P], F32, name="ident")
         w0_raw = keep.tile([P, 2 * N], U8, name="w0_raw", align_bytes=64)
-        w0s_raw = keep.tile([P, N], U8, name="w0s_raw", align_bytes=64)
         w0_perm = keep.tile([P, 2 * H], U8, name="w0_perm", align_bytes=64)
+        w0s_packed = keep.tile([P, PASS], U8, name="w0s_packed", align_bytes=64)
+        w0s_sorted = keep.tile([P, PASS], U8, name="w0s_sorted", align_bytes=64)
         w0s_perm = keep.tile([P, H], U8, name="w0s_perm", align_bytes=64)
+        w0s_out = keep.tile([P, OS], U8, name="w0s_out", align_bytes=64)
         w1 = keep.tile([P, G, 2 * OS], U8, name="w1", align_bytes=64)
         w1s = keep.tile([P, G, OS], U8, name="w1s", align_bytes=64)
         bias_h = keep.tile([P, G, T], BF16, name="bias_h")
@@ -71,7 +70,9 @@ def tile_spn_w4_kernel(tc, x_bytes, x_scale, w0_words, w0_scales, w1_words, w1_s
             raw = keep.tile([P, CHUNKS[c], X], U8, name="xbytes%d" % c, align_bytes=64)
             x_raw.append(raw)
 
-        nc.vector.memset(w0s_raw[:].bitcast(I32), 0)
+        nc.vector.memset(w0s_packed[P // 2 :].bitcast(I32), 0)
+        nc.vector.memset(w0s_perm[:].bitcast(I32), 0)
+        nc.vector.memset(w0s_out[:].bitcast(I32), 0)
         nc.vector.memset(w1s[:].rearrange("p g n -> p (g n)").bitcast(I32), 0)
         make_identity(nc, ident[:])
 
@@ -81,37 +82,8 @@ def tile_spn_w4_kernel(tc, x_bytes, x_scale, w0_words, w0_scales, w1_words, w1_s
         def load_w0(n0, n1):
             nc.sync.dma_start(out=w0_raw[:, 2 * n0 : 2 * n1], in_=w0_words[0, :, 2 * n0 : 2 * n1])
 
-        load_x(0)
-        nc.sync.dma_start(out=xs_col[:], in_=x_scale.rearrange("o (p t) -> p (o t)", t=T))
-        load_x(1)
-        load_w0(0, PASS)
-        for q in range(4):
-            nc.sync.dma_start(
-                out=w0s_raw[32 * q : 32 * q + 4, :].bitcast(I32),
-                in_=w0_scales[0, 4 * q : 4 * q + 4, :].bitcast(I32),
-            )
-        load_x(2)
-        nc.sync.dma_start(out=bias_h[:], in_=biases[0:H].rearrange("(g p t) -> p g t", g=G, p=P, t=T))
-        load_x(3)
-        load_w0(PASS, 2 * PASS)
-        load_w0(2 * PASS, N)
-        nc.sync.dma_start(out=w1[:], in_=w1_words.rearrange("g p n -> p g n"))
-        for q in range(4):
-            nc.sync.dma_start(
-                out=w1s[32 * q : 32 * q + 4].bitcast(I32),
-                in_=w1_scales[:, 4 * q : 4 * q + 4, :].rearrange("g r n -> r g n").bitcast(I32),
-            )
-        load_x(last)
-        nc.sync.dma_start(out=bias_o[:], in_=biases[H:N].partition_broadcast(P))
-
         x_wide, x_turned, x_woven, x_codes, x_scales = {}, {}, {}, {}, {}
-        z_kept, h_planes, h_woven, h_codes, h_scales, sums = {}, {}, {}, {}, {}, {}
-        side_turns = []
-
-        def side_bank():
-            side_turns.append(len(side_turns) % SIDE_BANKS)
-            return "side%d" % side_turns[-1]
-
+        h_planes, h_woven, h_codes, h_scales, sums, z_kept = {}, {}, {}, {}, {}, {}
 
         def permute_words(g0, g1):
             cols = slice(2 * PASS * g0, 2 * PASS * g1)
@@ -119,14 +91,6 @@ def tile_spn_w4_kernel(tc, x_bytes, x_scale, w0_words, w0_scales, w1_words, w1_s
                 out=w0_perm[:, cols].bitcast(U16).rearrange("p (g t m) -> p g t m", t=T, m=P),
                 in_=w0_raw[:, cols].bitcast(U16).rearrange("p (g m t) -> p g t m", t=T, m=P),
             )
-
-        def permute_scales(g0, g1):
-            cols = slice(PASS * g0, PASS * g1)
-            nc.vector.tensor_copy(
-                out=w0s_perm[:, cols].rearrange("p (g t m) -> p g t m", t=T, m=P),
-                in_=w0s_raw[:, cols].rearrange("p (g m t) -> p g t m", t=T, m=P),
-            )
-
 
         def x_cast(c, j0, count, cast):
             wide = keep.tile([P, count, X], BF16, name="xv%d_%d" % (c, j0), align_bytes=64)
@@ -140,8 +104,8 @@ def tile_spn_w4_kernel(tc, x_bytes, x_scale, w0_words, w0_scales, w1_words, w1_s
         def scalar_activation_cast(out, in_):
             nc.scalar.activation(out=out, in_=in_, func=COPY)
 
-        def x_transpose(c, j0, count):
-            bank = psum.tile([P, 2, count, P], F32, name="xt", tag=side_bank(), bufs=1)
+        def x_transpose(c, j0, count, tag):
+            bank = psum.tile([P, 2, count, P], F32, name="xt", tag=tag, bufs=1)
             x_turned[c, j0] = bank
             for jj in range(count):
                 words = x_wide[c, j0 + jj].bitcast(F32)
@@ -159,23 +123,19 @@ def tile_spn_w4_kernel(tc, x_bytes, x_scale, w0_words, w0_scales, w1_words, w1_s
                 op=MULT,
             )
 
-        def x_quantize(c):
-            n = CHUNKS[c] * P
-            x_codes[c] = work.tile([P, MAX_TOKENS], U32, name="xq", bufs=n_chunks, align_bytes=64)
-            x_scales[c] = work.tile([P, MAX_TOKENS], U8, name="xqs", bufs=n_chunks, align_bytes=64)
-            nc.vector.quantize_mx(out=x_codes[c][:, :n].bitcast(FP8X4), scales=x_scales[c][:, :n], in_=x_woven[c][:, : T * n])
+        def x_quantize(c, lo=0, hi=None):
+            hi = CHUNKS[c] * P if hi is None else hi
+            if lo == 0:
+                x_codes[c] = work.tile([P, MAX_TOKENS], U32, name="xq", bufs=n_chunks, align_bytes=64)
+                x_scales[c] = work.tile([P, MAX_TOKENS], U8, name="xqs", bufs=n_chunks, align_bytes=64)
+            nc.vector.quantize_mx(out=x_codes[c][:, lo:hi].bitcast(FP8X4), scales=x_scales[c][:, lo:hi], in_=x_woven[c][:, T * lo : T * hi])
 
-
-        def plane(k):
-            u, t = divmod(k, T)
+        def plane(u, t, z):
             c, g = divmod(u, G)
             n = tokens(u)
-            if t == 0:
-                h_planes[u] = work.tile([P, T, MAX_TOKENS + PLANE_PAD], BF16, name="hp", bufs=6, align_bytes=64)
-            z = psum.tile([P, MAX_TOKENS], F32, name="z", bufs=PLANE_BANKS)
             m0 = PASS * g + P * t
             nc.tensor.matmul_mx(
-                out=z[:, :n],
+                out=z,
                 lhsT=w0_perm[:, 2 * m0 : 2 * (m0 + P)].bitcast(FP4X4),
                 lhsT_scale=w0s_perm[:, m0 : m0 + P],
                 rhs=x_codes[c][:, :n].bitcast(FP8X4),
@@ -183,34 +143,51 @@ def tile_spn_w4_kernel(tc, x_bytes, x_scale, w0_words, w0_scales, w1_words, w1_s
                 start=True,
                 stop=True,
             )
-            if k == VECTOR_PLANE:
-                z_kept[k] = z
-            else:
-                nc.scalar.activation(out=h_planes[u][:, t, :n], in_=z[:, :n], func=RELU, bias=bias_h[:, g, t : t + 1])
 
-        def vector_plane_out(k):
-            u, t = divmod(k, T)
+        def per_bank(u):
+            return MAX_TOKENS // tokens(u) if u else 1
+
+        def fill_bank(u, t0):
             n = tokens(u)
-            nc.vector.tensor_scalar(
-                out=h_planes[u][:, t, :n], in0=z_kept[k][:, :n], scalar1=bias_h[:, u % G, t : t + 1], scalar2=0.0, op0=ADD, op1=MAX
-            )
+            count = per_bank(u)
+            if t0 == 0:
+                h_planes[u] = work.tile([P, T, MAX_TOKENS + PLANE_PAD], BF16, name="hp", bufs=6, align_bytes=64)
+            tag, bufs = ("o1", 1) if (u, t0) in VECTOR_BANKS else ("z", PLANE_BANKS)
+            bank = psum.tile([P, count, n], F32, name="z", tag=tag, bufs=bufs)
+            for i in range(count):
+                plane(u, t0 + i, bank[:, i, :])
+            if (u, t0) in VECTOR_BANKS:
+                z_kept[u, t0] = bank
+                return
+            for i in range(count):
+                t = t0 + i
+                nc.scalar.activation(out=h_planes[u][:, t, :n], in_=bank[:, i, :], func=RELU, bias=bias_h[:, u % G, t : t + 1])
 
-        def woven_tile(u, a, b, tag, bufs):
-            h_woven[u, a] = work.tile([P, T * (b - a)], BF16, name="hg", tag=tag, bufs=bufs, align_bytes=64)
+        def vector_bank_out(u, t0):
+            for i in range(per_bank(u)):
+                t = t0 + i
+                nc.vector.tensor_scalar(
+                    out=h_planes[u][:, t, : tokens(u)], in0=z_kept[u, t0][:, i, :], scalar1=bias_h[:, u % G, t : t + 1], scalar2=0.0, op0=ADD, op1=MAX
+                )
 
-        def weave(copy, u, a, lo, hi):
+        def woven_tile(u):
+            if u not in h_woven:
+                tag, bufs = ("odd%d" % (min(u, n_units - G - 1) // 2 % 2), 1) if u % 2 else ("even", 1)
+                h_woven[u] = work.tile([P, T * MAX_TOKENS], BF16, name="hg", tag=tag, bufs=bufs, align_bytes=64)
+            return h_woven[u]
+
+        def weave(copy, u, lo, hi):
             copy(
-                out=h_woven[u, a][:, T * (lo - a) : T * (hi - a)].rearrange("p (c i t) -> p c t i", t=T, i=4),
+                out=woven_tile(u)[:, T * lo : T * hi].rearrange("p (c i t) -> p c t i", t=T, i=4),
                 in_=h_planes[u][:, :, lo:hi].rearrange("p t (c i) -> p c t i", i=4),
             )
 
-        def weave_own(copy, u, a, b):
-            woven_tile(u, a, b, "hg", 4)
-            weave(copy, u, a, a, b)
+        def vector_weave(u):
+            weave(nc.vector.tensor_copy, u, 0, tokens(u))
 
-        def pool_weave(u, a, lo, hi):
+        def pool_weave(u, lo, hi):
             nc.gpsimd.tensor_scalar(
-                out=h_woven[u, a][:, T * (lo - a) : T * (hi - a)].rearrange("p (n t) -> p n t", t=T),
+                out=woven_tile(u)[:, T * lo : T * hi].rearrange("p (n t) -> p n t", t=T),
                 in0=h_planes[u][:, :, lo:hi].rearrange("p t n -> p n t"),
                 scalar1=1.0,
                 scalar2=0.0,
@@ -218,42 +195,37 @@ def tile_spn_w4_kernel(tc, x_bytes, x_scale, w0_words, w0_scales, w1_words, w1_s
                 op1=ADD,
             )
 
-        def h_quantize(u, a, b):
+        def h_quantize(u, lo=0, hi=None):
+            hi = tokens(u) if hi is None else hi
             if u not in h_codes:
-                h_codes[u] = work.tile([P, MAX_TOKENS], U32, name="hq", bufs=3 * G, align_bytes=64)
-                h_scales[u] = work.tile([P, MAX_TOKENS], U8, name="hqs", bufs=3 * G, align_bytes=64)
-            nc.vector.quantize_mx(out=h_codes[u][:, a:b].bitcast(FP8X4), scales=h_scales[u][:, a:b], in_=h_woven[u, a][:])
+                h_codes[u] = work.tile([P, MAX_TOKENS], U32, name="hq", bufs=2 * G, align_bytes=64)
+                h_scales[u] = work.tile([P, MAX_TOKENS], U8, name="hqs", bufs=2 * G, align_bytes=64)
+            nc.vector.quantize_mx(out=h_codes[u][:, lo:hi].bitcast(FP8X4), scales=h_scales[u][:, lo:hi], in_=h_woven[u][:, T * lo : T * hi])
 
-
-        def out_pass(dst, codes, scales, j, w, w_scales, start, stop):
+        def out_pass(c, j, codes, scales, w, w_scales, start, stop):
+            per_bank = 1 if c == last else 2
+            bank, place = divmod(j, per_bank)
+            if start and place == 0:
+                sums[c, bank] = psum.tile([P, per_bank, OS], F32, name="o", tag=("x%d" if c == last else "o%d") % bank, bufs=1)
             cols = slice(j * P, (j + 1) * P)
             nc.tensor.matmul_mx(
-                out=dst,
+                out=sums[c, bank][:, place, :],
                 lhsT=codes[:, cols].bitcast(FP8X4),
                 lhsT_scale=scales[:, cols],
                 rhs=w.bitcast(FP4X4),
                 rhs_scale=w_scales,
-                start=start,
-                stop=stop,
+                start=start and place == 0,
+                stop=stop and place == per_bank - 1,
             )
+
+        def slice_passes(c, tiles):
+            for j in tiles:
+                out_pass(c, j, x_codes[c], x_scales[c], w0_raw[:, 2 * H : 2 * N], w0s_out[:], True, False)
 
         def unit_passes(u, tiles):
             c, g = divmod(u, G)
-            per_bank = 1 if c == last else 2
             for j in tiles:
-                bank, place = divmod(j, per_bank)
-                if g == 0:
-                    if place == 0:
-                        tag, bufs = ("z", PLANE_BANKS) if c == last and j > 0 else (side_bank(), 1)
-                        sums[c, bank] = psum.tile([P, per_bank, OS], F32, name="o", tag=tag, bufs=bufs)
-                    w_out, w_out_scales = w0_raw[:, 2 * H : 2 * N], w0s_raw[:, H:N]
-                    out_pass(sums[c, bank][:, place, :], x_codes[c], x_scales[c], j, w_out, w_out_scales, place == 0, False)
-                closes = g == G - 1 and place == per_bank - 1
-                out_pass(sums[c, bank][:, place, :], h_codes[u], h_scales[u], j, w1[:, g, :], w1s[:, g, :], False, closes)
-
-        def pair_passes(c, pair):
-            for g in range(G):
-                unit_passes(G * c + g, (2 * pair, 2 * pair + 1))
+                out_pass(c, j, h_codes[u], h_scales[u], w1[:, g, :], w1s[:, g, :], False, g == G - 1)
 
         def store_pair(c, pair):
             res = work.tile([P, 2, OS], F32, name="res", bufs=4)
@@ -266,124 +238,166 @@ def tile_spn_w4_kernel(tc, x_bytes, x_scale, w0_words, w0_scales, w1_words, w1_s
             nc.vector.tensor_tensor(out=res[:], in0=sums[last, j][:, 0, :], in1=bias_o[:], op=ADD)
             nc.sync.dma_start(out=out_view[:, first_tile[last] + j, :], in_=res[:])
 
+        load_x(0)
+        nc.sync.dma_start(
+            out=w0s_packed[: P // 2].bitcast(I32),
+            in_=w0_scales[0, :, 0:H].rearrange("r (g n) -> r g n", g=G).bitcast(I32),
+        )
+        nc.sync.dma_start(out=xs_col[:], in_=x_scale.rearrange("o (p t) -> p (o t)", t=T))
+        load_w0(0, PASS)
+        load_x(1)
+        nc.sync.dma_start(out=bias_h[:], in_=biases[0:H].rearrange("(g p t) -> p g t", g=G, p=P, t=T))
+        load_w0(PASS, 2 * PASS)
+        load_x(2)
         x_cast(0, 0, 1, nc.vector.tensor_copy)
         x_cast(0, 1, 1, scalar_activation_cast)
-        x_transpose(0, 0, 1)
-        x_transpose(0, 1, 1)
-        x_cast(1, 0, 1, nc.vector.tensor_copy)
-        for j in range(1, CHUNKS[1]):
-            x_cast(1, j, 1, nc.scalar.copy)
+        nc.vector.tensor_copy(
+            out=w0s_sorted[:].rearrange("p (t m) -> p t m", t=T),
+            in_=w0s_packed[:].rearrange("p (m t) -> p t m", t=T),
+        )
+        for q in range(4):
+            nc.scalar.dma_start(
+                out=w0s_perm[32 * q : 32 * q + 4, :].bitcast(I32),
+                in_=w0s_sorted[16 * q : 16 * q + 16, :].bitcast(I32),
+            )
+        load_w0(2 * PASS, H)
+        load_x(3)
+        load_x(4)
+        load_w0(H, N)
+        nc.sync.dma_start(out=w1[:], in_=w1_words.rearrange("g p n -> p g n"))
+        for q in range(4):
+            nc.sync.dma_start(
+                out=w0s_out[32 * q : 32 * q + 4, :].bitcast(I32),
+                in_=w0_scales[0, 4 * q : 4 * q + 4, H:N].bitcast(I32),
+            )
+        for q in range(4):
+            nc.sync.dma_start(
+                out=w1s[32 * q : 32 * q + 4].bitcast(I32),
+                in_=w1_scales[:, 4 * q : 4 * q + 4, :].rearrange("g r n -> r g n").bitcast(I32),
+            )
+        nc.sync.dma_start(out=bias_o[:], in_=biases[H:N].partition_broadcast(P))
+
+        x_transpose(0, 0, 1, "o0")
+        x_transpose(0, 1, 1, "o1")
+        x_cast(1, 0, 2, nc.scalar.copy)
+        x_cast(1, 2, 2, nc.scalar.copy)
+        x_cast(2, 0, 4, nc.scalar.copy)
+
         permute_words(0, 1)
-        x_transpose(1, 0, 2)
+        x_transpose(1, 0, 2, "x0")
+        x_transpose(1, 2, 2, "x1")
         for j in range(CHUNKS[0]):
             x_scale_out(0, j, 1)
-        x_transpose(1, 2, 2)
-        x_cast(2, 0, 2, nc.scalar.copy)
-        x_cast(2, 2, 2, nc.scalar.copy)
-        x_cast(3, 0, 2, nc.scalar.copy)
-        permute_scales(0, 1)
-        x_quantize(0)
-        permute_scales(1, 2)
+        for j in range(CHUNKS[0]):
+            x_quantize(0, j * P, (j + 1) * P)
         permute_words(1, 2)
-        permute_scales(2, G)
+
         permute_words(2, G)
+        x_scale_out(1, 0, 2)
+        x_cast(3, 0, 2, nc.vector.tensor_copy)
+        x_quantize(1, 0, 2 * P)
 
+        behind = {}
 
-        def window_open(c):
+        def put(k, work_fn, *args):
+            behind.setdefault(k, []).append((work_fn, args))
+
+        def pairs(c):
+            return range(CHUNKS[c] // 2)
+
+        def pair_tiles(pair):
+            return (2 * pair, 2 * pair + 1)
+
+        slots = [(u, t) for u in range(n_units) for t in range(0, T, per_bank(u))]
+
+        def done(u):
+            return slots.index((u, T - per_bank(u)))
+
+        end = len(slots) - 1
+        for c in range(n_chunks):
             u = G * c
+            base = slots.index((u, 0))
             n = tokens(u)
             cut = n - POOL_TOKENS[c]
-            if c > 0:
-                h_quantize(u - 1, 0, tokens(u - 1))
-                pair_passes(c - 1, 0)
-            if 0 < c < last - 1:
-                x_cast(c + 2, CHUNKS[c + 2] - 2, 2, nc.vector.tensor_copy)
-                woven_tile(u, 0, n, "hand", 1)
-                pool_weave(u, 0, cut, n)
-            else:
+            window = base + 7 + LAG[c] if c else done(0)
+            if c < last:
+                put(window, pool_weave, u, cut, n)
+                for pair in pairs(c + 1)[0 if c else 1 :]:
+                    put(window, x_scale_out, c + 1, 2 * pair, 2)
+                k = window
+                if c > 0:
+                    put(window - 1, unit_passes, u - 2, range(CHUNKS[c - 1]))
+                    for pair in pairs(c - 1):
+                        k = window + pair
+                        put(k, unit_passes, u - 1, pair_tiles(pair))
+                        put(k, store_pair, c - 1, pair)
+                for vu, vt in VECTOR_BANKS:
+                    if vu // G == c:
+                        k = max(k, slots.index((vu, vt)))
+                        put(k, vector_bank_out, vu, vt)
                 if cut:
-                    weave_own(nc.vector.tensor_copy, u, 0, cut)
-                woven_tile(u, cut, n, "hand", 1)
-                pool_weave(u, cut, cut, n)
-            for j in range(0, CHUNKS[c + 1], 2):
-                x_scale_out(c + 1, j, 2)
-            if c > 0:
-                store_pair(c - 1, 0)
-
-        def window_close(c):
-            u = G * c
-            n = tokens(u)
-            cut = n - POOL_TOKENS[c]
-            if c == 0:
-                vector_plane_out(VECTOR_PLANE)
-            if 0 < c < last - 1:
-                weave(nc.vector.tensor_copy, u, 0, 0, cut)
-                x_quantize(c + 1)
-                h_quantize(u, 0, n)
+                    put(k, weave, nc.vector.tensor_copy, u, 0, cut)
+                if c == 0:
+                    put(k, x_quantize, 1, 2 * P, 4 * P)
+                else:
+                    put(k, x_quantize, c + 1)
+                put(k, h_quantize, u)
+                k = max(k, done(u + 1))
+                put(k, vector_weave, u + 1)
+                k = max(k, done(u + 2))
+                put(k, vector_weave, u + 2)
+                put(k, h_quantize, u + 1)
+                k = max(k, done(u + 3))
+                if c == 0:
+                    put(k, x_cast, 3, 2, 2, nc.vector.tensor_copy)
+                    put(k, x_cast, 4, 0, 2, nc.vector.tensor_copy)
+                if c + 1 < last:
+                    put(k, vector_weave, u + 3)
+                    put(k, h_quantize, u + 2)
+                    put(k, h_quantize, u + 3)
+                else:
+                    put(k, h_quantize, u + 2)
+                    put(k, vector_weave, u + 3)
+                if c + 2 < n_chunks:
+                    for pair in pairs(c + 2):
+                        put(window + (5 + 4 * pair if c == 0 else 4 + 2 * pair), x_transpose, c + 2, 2 * pair, 2, "x%d" % pair)
+                first = window + (4 if c == 0 else 7)
+                for pair in pairs(c):
+                    put(first + pair, slice_passes, c, pair_tiles(pair))
+                    put(window + (10 if c == 0 else 9) + pair, unit_passes, u, pair_tiles(pair))
+                    put(window + (12 if c == 0 else 13) + pair, unit_passes, u + 1, pair_tiles(pair))
             else:
-                if cut:
-                    h_quantize(u, 0, cut)
-                x_quantize(c + 1)
-                h_quantize(u, cut, n)
+                put(base + 2, slice_passes, c, (0, 1))
 
-        def plain_step(u):
-            c, g = divmod(u, G)
-            n = tokens(u)
-            if g == G - 1 and c + 1 < last:
-                woven_tile(u, 0, n, "hand", 1)
-                weave(nc.vector.tensor_copy, u, 0, 0, n)
-            elif u in scalar_tokens:
-                weave(nc.vector.tensor_copy, u, 0, 0, n - scalar_tokens[u])
-            else:
-                weave_own(nc.vector.tensor_copy, u, 0, n)
-            if g > 1 or u > last_start:
-                h_quantize(u - 1, 0, tokens(u - 1))
-            if u == last_start - 1:
-                h_quantize(u, 0, n)
-            if g == G - 1 and 0 < c < last and CHUNKS[c - 1] > 2:
-                store_pair(c - 1, 1)
-            if u == last_start + 1:
-                store_pair(last - 1, 0)
+                put(done(u) + 1, weave, nc.vector.tensor_copy, u, 0, n - 0)
+                for pair in pairs(c - 1):
+                    put(done(u) + 1, h_quantize, u - 1, 2 * P * pair, 2 * P * (pair + 1))
+                put(done(u) + 1, h_quantize, u)
+                for pair in pairs(c - 1):
+                    put(base + 4 + pair, unit_passes, u - 2, pair_tiles(pair))
+                put(end, pool_weave, u + 1, cut, n)
+                put(end, weave, nc.vector.tensor_copy, u + 1, 0, cut)
+                for pair in pairs(c - 1):
+                    put(end - 1 + pair, unit_passes, u - 1, pair_tiles(pair))
+                put(end, store_pair, c - 1, 0)
+                put(end, unit_passes, u, (0, 1))
+                put(end, vector_weave, u + 2)
+                put(end, h_quantize, u + 1)
+                put(end, unit_passes, u + 1, (0, 1))
+                woven_last = work.tile([P, T * MAX_TOKENS], BF16, name="hg", tag="last", bufs=1, align_bytes=64)
+                h_woven[u + 3] = woven_last
+                put(end, weave, nc.vector.tensor_copy, u + 3, 0, P)
+                put(end, weave, nc.scalar.copy, u + 3, P, 2 * P)
+                put(end, h_quantize, u + 2)
+                put(end, unit_passes, u + 2, (0, 1))
+                for j in range(CHUNKS[c]):
+                    put(end, h_quantize, u + 3, j * P, (j + 1) * P)
+                    put(end, unit_passes, u + 3, (j,))
+                put(end, store_pair, c - 1, 1)
+                for j in range(CHUNKS[c]):
+                    put(end, store_last, j)
 
-        def last_step(u):
-            weave_own(nc.vector.tensor_copy, u, 0, P)
-            weave_own(nc.scalar.copy, u, P, 2 * P)
-            h_quantize(u - 1, 0, tokens(u - 1))
-            unit_passes(u - 1, range(CHUNKS[last]))
-            for j in range(CHUNKS[last]):
-                h_quantize(u, j * P, (j + 1) * P)
-                unit_passes(u, (j,))
-            store_pair(last - 1, 1)
-            for j in range(CHUNKS[last]):
-                store_last(j)
-
-        def step_plane(u):
-            return T * (u + 1) + PLANE_BANKS
-
-        n_planes = T * n_units
-        for k in range(step_plane(n_units - 1) + 1):
-            c, place = divmod(k, T * G)
-            if k < n_planes:
-                plane(k)
-            for u in scalar_tokens:
-                if k == T * (u + 1):
-                    woven_tile(u, 0, tokens(u), "hs", 3)
-                    weave(nc.scalar.copy, u, 0, tokens(u) - scalar_tokens[u], tokens(u))
-            if place == 2 and 0 < c < last:
-                for j in range(0, CHUNKS[c + 1], 2):
-                    x_transpose(c + 1, j, 2)
-            if k == step_plane(G * c + 1) and 0 < c < last and CHUNKS[c - 1] > 2:
-                pair_passes(c - 1, 1)
-            for u in range(last_start - G, n_units - 2):
-                if k == min(step_plane(u + 2), step_plane(n_units - 2) + 1):
-                    unit_passes(u, range(CHUNKS[u // G]))
-            for u in range(n_units):
-                if k == step_plane(u):
-                    if u == n_units - 1:
-                        last_step(u)
-                    elif u % G == 0 and u < last_start:
-                        window_open(u // G)
-                    else:
-                        plain_step(u)
-            if c < last and k == (VECTOR_PLANE if c == 0 else step_plane(G * c)):
-                window_close(c)
+        for k, (u, t) in enumerate(slots):
+            fill_bank(u, t)
+            for work_fn, args in behind.get(k, []):
+                work_fn(*args)

@@ -29,7 +29,7 @@ FLOPS = 2 * B * X * N + 2 * B * H * OS
 CHUNKS = (2, 4, 4, 4, 2)
 MAX_TOKENS = max(CHUNKS) * P
 PLANE_BANKS = 4
-POOL_TOKENS = (256, 480, 512, 384, 96)
+POOL_TOKENS = (256, 416, 512, 352, 0)
 LAG = (0, 0, 0, 0, 0)
 PLANE_PAD = 16
 VECTOR_BANKS = ((2, 0),)
@@ -56,10 +56,8 @@ def tile_spn_w4_kernel(tc, x_bytes, x_scale, w0_words, w0_scales, w1_words, w1_s
         ident = keep.tile([P, P], F32, name="ident")
         w0_raw = keep.tile([P, 2 * N], U8, name="w0_raw", align_bytes=64)
         w0_perm = keep.tile([P, 2 * H], U8, name="w0_perm", align_bytes=64)
-        w0s_packed = keep.tile([P, PASS], U8, name="w0s_packed", align_bytes=64)
-        w0s_sorted = keep.tile([P, PASS], U8, name="w0s_sorted", align_bytes=64)
+        w0s_raw = keep.tile([P, N], U8, name="w0s_raw", align_bytes=64)
         w0s_perm = keep.tile([P, H], U8, name="w0s_perm", align_bytes=64)
-        w0s_out = keep.tile([P, OS], U8, name="w0s_out", align_bytes=64)
         w1 = keep.tile([P, G, 2 * OS], U8, name="w1", align_bytes=64)
         w1s = keep.tile([P, G, OS], U8, name="w1s", align_bytes=64)
         bias_h = keep.tile([P, G, T], BF16, name="bias_h")
@@ -70,9 +68,7 @@ def tile_spn_w4_kernel(tc, x_bytes, x_scale, w0_words, w0_scales, w1_words, w1_s
             raw = keep.tile([P, CHUNKS[c], X], U8, name="xbytes%d" % c, align_bytes=64)
             x_raw.append(raw)
 
-        nc.vector.memset(w0s_packed[P // 2 :].bitcast(I32), 0)
-        nc.vector.memset(w0s_perm[:].bitcast(I32), 0)
-        nc.vector.memset(w0s_out[:].bitcast(I32), 0)
+        nc.vector.memset(w0s_raw[:].bitcast(I32), 0)
         nc.vector.memset(w1s[:].rearrange("p g n -> p (g n)").bitcast(I32), 0)
         make_identity(nc, ident[:])
 
@@ -85,11 +81,18 @@ def tile_spn_w4_kernel(tc, x_bytes, x_scale, w0_words, w0_scales, w1_words, w1_s
         x_wide, x_turned, x_woven, x_codes, x_scales = {}, {}, {}, {}, {}
         h_planes, h_woven, h_codes, h_scales, sums, z_kept = {}, {}, {}, {}, {}, {}
 
-        def permute_words(g0, g1):
+        def permute_words(g0, g1, copy=nc.vector.tensor_copy):
             cols = slice(2 * PASS * g0, 2 * PASS * g1)
-            nc.vector.tensor_copy(
+            copy(
                 out=w0_perm[:, cols].bitcast(U16).rearrange("p (g t m) -> p g t m", t=T, m=P),
                 in_=w0_raw[:, cols].bitcast(U16).rearrange("p (g m t) -> p g t m", t=T, m=P),
+            )
+
+        def permute_scales(g0, g1):
+            cols = slice(PASS * g0, PASS * g1)
+            nc.vector.tensor_copy(
+                out=w0s_perm[:, cols].rearrange("p (g t m) -> p g t m", t=T, m=P),
+                in_=w0s_raw[:, cols].rearrange("p (g m t) -> p g t m", t=T, m=P),
             )
 
         def x_cast(c, j0, count, cast):
@@ -113,11 +116,15 @@ def tile_spn_w4_kernel(tc, x_bytes, x_scale, w0_words, w0_scales, w1_words, w1_s
                     nc.tensor.transpose(bank[:, u, jj, :], words[:, u : X // 2 : 2], ident[:])
 
         def x_scale_out(c, j0, count):
-            if j0 == 0:
-                x_woven[c] = work.tile([P, T * MAX_TOKENS], BF16, name="xg", bufs=2, align_bytes=64)
+            if (c, j0) == (1, 0):
+                x_woven[c, j0] = work.tile([P, T * MAX_TOKENS], BF16, name="xg", tag="even", bufs=1, align_bytes=64)
+            elif j0 == 0 or c == 1:
+                x_woven[c, j0] = work.tile([P, T * MAX_TOKENS], BF16, name="xg", bufs=2, align_bytes=64)
+            else:
+                x_woven[c, j0] = x_woven[c, 0]
             halves = x_turned[c, j0][:].rearrange("p u j r -> p (u j r)").bitcast(BF16)
             nc.vector.tensor_tensor(
-                out=x_woven[c][:, T * P * j0 : T * P * (j0 + count)].rearrange("p (r u e) -> p r u e", u=2, e=2),
+                out=x_woven[c, j0][:, T * P * j0 : T * P * (j0 + count)].rearrange("p (r u e) -> p r u e", u=2, e=2),
                 in0=halves.rearrange("p (u r e) -> p r u e", u=2, e=2),
                 in1=xs_col[:].rearrange("p (o u e) -> p o u e", o=1, u=2).to_broadcast([P, count * P, 2, 2]),
                 op=MULT,
@@ -128,7 +135,7 @@ def tile_spn_w4_kernel(tc, x_bytes, x_scale, w0_words, w0_scales, w1_words, w1_s
             if lo == 0:
                 x_codes[c] = work.tile([P, MAX_TOKENS], U32, name="xq", bufs=n_chunks, align_bytes=64)
                 x_scales[c] = work.tile([P, MAX_TOKENS], U8, name="xqs", bufs=n_chunks, align_bytes=64)
-            nc.vector.quantize_mx(out=x_codes[c][:, lo:hi].bitcast(FP8X4), scales=x_scales[c][:, lo:hi], in_=x_woven[c][:, T * lo : T * hi])
+            nc.vector.quantize_mx(out=x_codes[c][:, lo:hi].bitcast(FP8X4), scales=x_scales[c][:, lo:hi], in_=x_woven[c, lo // P][:, T * lo : T * hi])
 
         def plane(u, t, z):
             c, g = divmod(u, G)
@@ -220,7 +227,7 @@ def tile_spn_w4_kernel(tc, x_bytes, x_scale, w0_words, w0_scales, w1_words, w1_s
 
         def slice_passes(c, tiles):
             for j in tiles:
-                out_pass(c, j, x_codes[c], x_scales[c], w0_raw[:, 2 * H : 2 * N], w0s_out[:], True, False)
+                out_pass(c, j, x_codes[c], x_scales[c], w0_raw[:, 2 * H : 2 * N], w0s_raw[:, H:N], True, False)
 
         def unit_passes(u, tiles):
             c, g = divmod(u, G)
@@ -239,37 +246,24 @@ def tile_spn_w4_kernel(tc, x_bytes, x_scale, w0_words, w0_scales, w1_words, w1_s
             nc.sync.dma_start(out=out_view[:, first_tile[last] + j, :], in_=res[:])
 
         load_x(0)
-        nc.sync.dma_start(
-            out=w0s_packed[: P // 2].bitcast(I32),
-            in_=w0_scales[0, :, 0:H].rearrange("r (g n) -> r g n", g=G).bitcast(I32),
-        )
         nc.sync.dma_start(out=xs_col[:], in_=x_scale.rearrange("o (p t) -> p (o t)", t=T))
         load_w0(0, PASS)
         load_x(1)
-        nc.sync.dma_start(out=bias_h[:], in_=biases[0:H].rearrange("(g p t) -> p g t", g=G, p=P, t=T))
-        load_w0(PASS, 2 * PASS)
+        for q in range(4):
+            nc.sync.dma_start(
+                out=w0s_raw[32 * q : 32 * q + 4, :].bitcast(I32),
+                in_=w0_scales[0, 4 * q : 4 * q + 4, :].bitcast(I32),
+            )
         load_x(2)
+        load_w0(PASS, 2 * PASS)
+        nc.sync.dma_start(out=bias_h[:], in_=biases[0:H].rearrange("(g p t) -> p g t", g=G, p=P, t=T))
         x_cast(0, 0, 1, nc.vector.tensor_copy)
         x_cast(0, 1, 1, scalar_activation_cast)
-        nc.vector.tensor_copy(
-            out=w0s_sorted[:].rearrange("p (t m) -> p t m", t=T),
-            in_=w0s_packed[:].rearrange("p (m t) -> p t m", t=T),
-        )
-        for q in range(4):
-            nc.scalar.dma_start(
-                out=w0s_perm[32 * q : 32 * q + 4, :].bitcast(I32),
-                in_=w0s_sorted[16 * q : 16 * q + 16, :].bitcast(I32),
-            )
         load_w0(2 * PASS, H)
         load_x(3)
         load_x(4)
         load_w0(H, N)
         nc.sync.dma_start(out=w1[:], in_=w1_words.rearrange("g p n -> p g n"))
-        for q in range(4):
-            nc.sync.dma_start(
-                out=w0s_out[32 * q : 32 * q + 4, :].bitcast(I32),
-                in_=w0_scales[0, 4 * q : 4 * q + 4, H:N].bitcast(I32),
-            )
         for q in range(4):
             nc.sync.dma_start(
                 out=w1s[32 * q : 32 * q + 4].bitcast(I32),
@@ -288,14 +282,15 @@ def tile_spn_w4_kernel(tc, x_bytes, x_scale, w0_words, w0_scales, w1_words, w1_s
         x_transpose(1, 2, 2, "x1")
         for j in range(CHUNKS[0]):
             x_scale_out(0, j, 1)
-        for j in range(CHUNKS[0]):
-            x_quantize(0, j * P, (j + 1) * P)
-        permute_words(1, 2)
-
-        permute_words(2, G)
+        permute_scales(0, 1)
+        x_quantize(0)
+        permute_scales(1, 2)
+        permute_words(1, 2, nc.scalar.copy)
         x_scale_out(1, 0, 2)
-        x_cast(3, 0, 2, nc.vector.tensor_copy)
+        permute_scales(2, G)
+        permute_words(2, 3)
         x_quantize(1, 0, 2 * P)
+        permute_words(3, G)
 
         behind = {}
 
@@ -314,6 +309,7 @@ def tile_spn_w4_kernel(tc, x_bytes, x_scale, w0_words, w0_scales, w1_words, w1_s
             return slots.index((u, T - per_bank(u)))
 
         end = len(slots) - 1
+        put(9, x_cast, 4, 0, 2, nc.scalar.copy)
         for c in range(n_chunks):
             u = G * c
             base = slots.index((u, 0))
@@ -349,8 +345,7 @@ def tile_spn_w4_kernel(tc, x_bytes, x_scale, w0_words, w0_scales, w1_words, w1_s
                 put(k, h_quantize, u + 1)
                 k = max(k, done(u + 3))
                 if c == 0:
-                    put(k, x_cast, 3, 2, 2, nc.vector.tensor_copy)
-                    put(k, x_cast, 4, 0, 2, nc.vector.tensor_copy)
+                    put(k, x_cast, 3, 0, 4, nc.vector.tensor_copy)
                 if c + 1 < last:
                     put(k, vector_weave, u + 3)
                     put(k, h_quantize, u + 2)
@@ -375,7 +370,6 @@ def tile_spn_w4_kernel(tc, x_bytes, x_scale, w0_words, w0_scales, w1_words, w1_s
                 put(done(u) + 1, h_quantize, u)
                 for pair in pairs(c - 1):
                     put(base + 4 + pair, unit_passes, u - 2, pair_tiles(pair))
-                put(end, pool_weave, u + 1, cut, n)
                 put(end, weave, nc.vector.tensor_copy, u + 1, 0, cut)
                 for pair in pairs(c - 1):
                     put(end - 1 + pair, unit_passes, u - 1, pair_tiles(pair))

@@ -29,10 +29,10 @@ FLOPS = 2 * B * X * N + 2 * B * H * OS
 CHUNKS = (2, 4, 4, 4, 2)
 MAX_TOKENS = max(CHUNKS) * P
 PLANE_BANKS = 4
-POOL_TOKENS = (256, 416, 512, 352, 0)
-LAG = (0, 0, 0, 0, 0)
+POOL_TOKENS = (256, 512, 512, 352)
 PLANE_PAD = 16
-VECTOR_BANKS = ((2, 0),)
+VECTOR_UNITS = (3, 6,)
+HALF = MAX_TOKENS // 2
 
 
 def tile_spn_w4_kernel(tc, x_bytes, x_scale, w0_words, w0_scales, w1_words, w1_scales, biases, out):
@@ -79,7 +79,7 @@ def tile_spn_w4_kernel(tc, x_bytes, x_scale, w0_words, w0_scales, w1_words, w1_s
             nc.sync.dma_start(out=w0_raw[:, 2 * n0 : 2 * n1], in_=w0_words[0, :, 2 * n0 : 2 * n1])
 
         x_wide, x_turned, x_woven, x_codes, x_scales = {}, {}, {}, {}, {}
-        h_planes, h_woven, h_codes, h_scales, sums, z_kept = {}, {}, {}, {}, {}, {}
+        h_planes, h_woven, h_codes, h_scales, sums, z_kept, h_pairs = {}, {}, {}, {}, {}, {}, {}
 
         def permute_words(g0, g1, copy=nc.vector.tensor_copy):
             cols = slice(2 * PASS * g0, 2 * PASS * g1)
@@ -105,7 +105,8 @@ def tile_spn_w4_kernel(tc, x_bytes, x_scale, w0_words, w0_scales, w1_words, w1_s
             )
 
         def scalar_activation_cast(out, in_):
-            nc.scalar.activation(out=out, in_=in_, func=COPY)
+            nc.scalar.activation(out=out[:, :P], in_=in_[:, :P], func=COPY)
+            nc.scalar.copy(out=out[:, P:], in_=in_[:, P:])
 
         def x_transpose(c, j0, count, tag):
             bank = psum.tile([P, 2, count, P], F32, name="xt", tag=tag, bufs=1)
@@ -137,49 +138,66 @@ def tile_spn_w4_kernel(tc, x_bytes, x_scale, w0_words, w0_scales, w1_words, w1_s
                 x_scales[c] = work.tile([P, MAX_TOKENS], U8, name="xqs", bufs=n_chunks, align_bytes=64)
             nc.vector.quantize_mx(out=x_codes[c][:, lo:hi].bitcast(FP8X4), scales=x_scales[c][:, lo:hi], in_=x_woven[c, lo // P][:, T * lo : T * hi])
 
-        def plane(u, t, z):
+        def plane(u, t, lo, z):
             c, g = divmod(u, G)
-            n = tokens(u)
             m0 = PASS * g + P * t
+            cols = slice(lo, lo + z.shape[1])
             nc.tensor.matmul_mx(
                 out=z,
                 lhsT=w0_perm[:, 2 * m0 : 2 * (m0 + P)].bitcast(FP4X4),
                 lhsT_scale=w0s_perm[:, m0 : m0 + P],
-                rhs=x_codes[c][:, :n].bitcast(FP8X4),
-                rhs_scale=x_scales[c][:, :n],
+                rhs=x_codes[c][:, cols].bitcast(FP8X4),
+                rhs_scale=x_scales[c][:, cols],
                 start=True,
                 stop=True,
             )
 
-        def per_bank(u):
-            return MAX_TOKENS // tokens(u) if u else 1
+        def scalar_tokens(u):
+            return tokens(u) - HALF if u in VECTOR_UNITS else tokens(u)
 
-        def fill_bank(u, t0):
-            n = tokens(u)
-            count = per_bank(u)
+        def per_bank(u):
+            return MAX_TOKENS // scalar_tokens(u) if u else 1
+
+        def scalar_bank(u, t0):
+            n, count = scalar_tokens(u), per_bank(u)
             if t0 == 0:
                 h_planes[u] = work.tile([P, T, MAX_TOKENS + PLANE_PAD], BF16, name="hp", bufs=6, align_bytes=64)
-            tag, bufs = ("o1", 1) if (u, t0) in VECTOR_BANKS else ("z", PLANE_BANKS)
-            bank = psum.tile([P, count, n], F32, name="z", tag=tag, bufs=bufs)
+            bank = psum.tile([P, count, n], F32, name="z", bufs=PLANE_BANKS)
             for i in range(count):
-                plane(u, t0 + i, bank[:, i, :])
-            if (u, t0) in VECTOR_BANKS:
-                z_kept[u, t0] = bank
-                return
+                plane(u, t0 + i, 0, bank[:, i, :])
             for i in range(count):
                 t = t0 + i
                 nc.scalar.activation(out=h_planes[u][:, t, :n], in_=bank[:, i, :], func=RELU, bias=bias_h[:, u % G, t : t + 1])
 
-        def vector_bank_out(u, t0):
-            for i in range(per_bank(u)):
-                t = t0 + i
-                nc.vector.tensor_scalar(
-                    out=h_planes[u][:, t, : tokens(u)], in0=z_kept[u, t0][:, i, :], scalar1=bias_h[:, u % G, t : t + 1], scalar2=0.0, op0=ADD, op1=MAX
-                )
+        def vector_bank(u, half, tag):
+            bank = psum.tile([P, 2, HALF], F32, name="zv", tag=tag, bufs=1)
+            z_kept[u, half] = bank
+            for e in range(2):
+                plane(u, 2 * half + e, scalar_tokens(u), bank[:, e, :])
+
+        def vector_bank_out(u, half):
+            if half == 0:
+                h_pairs[u] = work.tile([P, 2, HALF, 2], BF16, name="hpair", bufs=1, align_bytes=64)
+            nc.vector.tensor_tensor(
+                out=h_pairs[u][:, half],
+                in0=z_kept[u, half][:].rearrange("p e n -> p n e"),
+                in1=bias_h[:, u % G, 2 * half : 2 * half + 2].unsqueeze(1).to_broadcast([P, HALF, 2]),
+                op=ADD,
+            )
+
+        def pairs_relu(u):
+            lo = scalar_tokens(u)
+            nc.vector.tensor_scalar(
+                out=woven_tile(u)[:, T * lo : T * (lo + HALF)].rearrange("p (n h e) -> p n h e", h=2, e=2),
+                in0=h_pairs[u][:].rearrange("p h n e -> p n h e"),
+                scalar1=0.0,
+                scalar2=None,
+                op0=MAX,
+            )
 
         def woven_tile(u):
             if u not in h_woven:
-                tag, bufs = ("odd%d" % (min(u, n_units - G - 1) // 2 % 2), 1) if u % 2 else ("even", 1)
+                tag, bufs = ("odd", 2) if u % 2 else ("even", 1)
                 h_woven[u] = work.tile([P, T * MAX_TOKENS], BF16, name="hg", tag=tag, bufs=bufs, align_bytes=64)
             return h_woven[u]
 
@@ -190,7 +208,10 @@ def tile_spn_w4_kernel(tc, x_bytes, x_scale, w0_words, w0_scales, w1_words, w1_s
             )
 
         def vector_weave(u):
-            weave(nc.vector.tensor_copy, u, 0, tokens(u))
+            if u in VECTOR_UNITS:
+                pairs_relu(u)
+            if scalar_tokens(u):
+                weave(nc.vector.tensor_copy, u, 0, scalar_tokens(u))
 
         def pool_weave(u, lo, hi):
             nc.gpsimd.tensor_scalar(
@@ -303,95 +324,115 @@ def tile_spn_w4_kernel(tc, x_bytes, x_scale, w0_words, w0_scales, w1_words, w1_s
         def pair_tiles(pair):
             return (2 * pair, 2 * pair + 1)
 
-        slots = [(u, t) for u in range(n_units) for t in range(0, T, per_bank(u))]
+        slots = [(u, t) for u in range(n_units) if scalar_tokens(u) for t in range(0, T, per_bank(u))]
 
         def done(u):
-            return slots.index((u, T - per_bank(u)))
+            return max(k for k, slot in enumerate(slots) if slot[0] <= u)
 
         end = len(slots) - 1
-        put(9, x_cast, 4, 0, 2, nc.scalar.copy)
-        for c in range(n_chunks):
+
+        k = done(0)
+        put(k, pool_weave, 0, 0, tokens(0))
+        put(k, x_scale_out, 1, 2, 2)
+        k = done(2) - 1
+        for half in range(2):
+            put(k, vector_bank, 3, half, "o%d" % half)
+        put(k, vector_bank_out, 3, 0)
+        put(k, x_quantize, 1, HALF, 2 * HALF)
+        put(k, vector_bank_out, 3, 1)
+        put(k, h_quantize, 0)
+        k = done(2)
+        put(k, vector_weave, 1)
+        put(k, vector_weave, 2)
+        put(k, h_quantize, 1)
+
+
+        put(k, vector_weave, 3)
+        put(k, h_quantize, 2)
+        put(k, h_quantize, 3)
+        put(done(2) + 0, x_transpose, 2, 0, 2, "x0")
+        put(done(2) + 3, x_transpose, 2, 2, 2, "x1")
+        put(done(2) + 4, slice_passes, 0, (0, 1))
+        put(done(2) + 5, unit_passes, 0, (0, 1))
+        put(done(2) + 6, unit_passes, 1, (0, 1))
+
+        put(done(2), x_cast, 3, 0, 2, nc.scalar.copy)
+        put(done(4), x_cast, 3, 2, 2, nc.scalar.copy)
+        put(done(8), x_cast, 4, 0, 2, nc.scalar.copy)
+        for c in range(1, last):
             u = G * c
-            base = slots.index((u, 0))
             n = tokens(u)
             cut = n - POOL_TOKENS[c]
-            window = base + 7 + LAG[c] if c else done(0)
-            if c < last:
-                put(window, pool_weave, u, cut, n)
-                for pair in pairs(c + 1)[0 if c else 1 :]:
-                    put(window, x_scale_out, c + 1, 2 * pair, 2)
-                k = window
-                if c > 0:
-                    put(window - 1, unit_passes, u - 2, range(CHUNKS[c - 1]))
-                    for pair in pairs(c - 1):
-                        k = window + pair
-                        put(k, unit_passes, u - 1, pair_tiles(pair))
-                        put(k, store_pair, c - 1, pair)
-                for vu, vt in VECTOR_BANKS:
-                    if vu // G == c:
-                        k = max(k, slots.index((vu, vt)))
-                        put(k, vector_bank_out, vu, vt)
-                if cut:
-                    put(k, weave, nc.vector.tensor_copy, u, 0, cut)
-                if c == 0:
-                    put(k, x_quantize, 1, 2 * P, 4 * P)
-                else:
-                    put(k, x_quantize, c + 1)
-                put(k, h_quantize, u)
-                k = max(k, done(u + 1))
-                put(k, vector_weave, u + 1)
-                k = max(k, done(u + 2))
-                put(k, vector_weave, u + 2)
-                put(k, h_quantize, u + 1)
-                k = max(k, done(u + 3))
-                if c == 0:
-                    put(k, x_cast, 3, 0, 4, nc.vector.tensor_copy)
-                if c + 1 < last:
-                    put(k, vector_weave, u + 3)
-                    put(k, h_quantize, u + 2)
-                    put(k, h_quantize, u + 3)
-                else:
-                    put(k, h_quantize, u + 2)
-                    put(k, vector_weave, u + 3)
-                if c + 2 < n_chunks:
-                    for pair in pairs(c + 2):
-                        put(window + (5 + 4 * pair if c == 0 else 4 + 2 * pair), x_transpose, c + 2, 2 * pair, 2, "x%d" % pair)
-                first = window + (4 if c == 0 else 7)
-                for pair in pairs(c):
-                    put(first + pair, slice_passes, c, pair_tiles(pair))
-                    put(window + (10 if c == 0 else 9) + pair, unit_passes, u, pair_tiles(pair))
-                    put(window + (12 if c == 0 else 13) + pair, unit_passes, u + 1, pair_tiles(pair))
+            window = done(u) + 4
+            put(window - 1, unit_passes, u - 2, range(CHUNKS[c - 1]))
+            put(window, pool_weave, u, cut, n)
+            for pair in pairs(c + 1):
+                put(window, x_scale_out, c + 1, 2 * pair, 2)
+            for pair in pairs(c - 1):
+                k = window + pair
+                put(k, unit_passes, u - 1, pair_tiles(pair))
+                put(k, store_pair, c - 1, pair)
+            if u + 2 in VECTOR_UNITS:
+                free = "x1" if c + 1 == last else "o1"
+                put(window - 0, vector_bank, u + 2, 0, free)
+                k = window + 2
+                put(k, vector_bank, u + 2, 1, "x0")
+                for half in range(2):
+                    put(k, vector_bank_out, u + 2, half)
+            if cut:
+                put(k, weave, nc.vector.tensor_copy, u, 0, cut)
+            put(k, x_quantize, c + 1)
+            put(k, h_quantize, u)
+            k = max(k, done(u + 1))
+            put(k, vector_weave, u + 1)
+            k = max(k, done(u + 2))
+            put(k, vector_weave, u + 2)
+            put(k, h_quantize, u + 1)
+            k = max(k, done(u + 3))
+            short = 2 if u + 2 in VECTOR_UNITS else 0
+            if c + 1 < last:
+                put(k, vector_weave, u + 3)
+                put(k, h_quantize, u + 2)
+                put(k, h_quantize, u + 3)
+                for pair in pairs(c + 2):
+                    put(window + 5 + 2 * pair, x_transpose, c + 2, 2 * pair, 2, "x%d" % pair)
             else:
-                put(base + 2, slice_passes, c, (0, 1))
+                put(k, h_quantize, u + 2)
+                put(k, vector_weave, u + 3)
+            for pair in pairs(c):
+                put(window + 7 + pair, slice_passes, c, pair_tiles(pair))
+                put(window + 9 + pair, unit_passes, u, pair_tiles(pair))
+                put(window + 13 - short + pair, unit_passes, u + 1, pair_tiles(pair))
 
-                put(done(u) + 1, weave, nc.vector.tensor_copy, u, 0, n - 0)
-                for pair in pairs(c - 1):
-                    put(done(u) + 1, h_quantize, u - 1, 2 * P * pair, 2 * P * (pair + 1))
-                put(done(u) + 1, h_quantize, u)
-                for pair in pairs(c - 1):
-                    put(base + 4 + pair, unit_passes, u - 2, pair_tiles(pair))
-                put(end, weave, nc.vector.tensor_copy, u + 1, 0, cut)
-                for pair in pairs(c - 1):
-                    put(end - 1 + pair, unit_passes, u - 1, pair_tiles(pair))
-                put(end, store_pair, c - 1, 0)
-                put(end, unit_passes, u, (0, 1))
-                put(end, vector_weave, u + 2)
-                put(end, h_quantize, u + 1)
-                put(end, unit_passes, u + 1, (0, 1))
-                woven_last = work.tile([P, T * MAX_TOKENS], BF16, name="hg", tag="last", bufs=1, align_bytes=64)
-                h_woven[u + 3] = woven_last
-                put(end, weave, nc.vector.tensor_copy, u + 3, 0, P)
-                put(end, weave, nc.scalar.copy, u + 3, P, 2 * P)
-                put(end, h_quantize, u + 2)
-                put(end, unit_passes, u + 2, (0, 1))
-                for j in range(CHUNKS[c]):
-                    put(end, h_quantize, u + 3, j * P, (j + 1) * P)
-                    put(end, unit_passes, u + 3, (j,))
-                put(end, store_pair, c - 1, 1)
-                for j in range(CHUNKS[c]):
-                    put(end, store_last, j)
+        c, u = last, last * G
+        base = done(u - 1) + 1
+        put(base + 2, slice_passes, c, (0, 1))
+        put(done(u) + 1, vector_weave, u)
+        for pair in pairs(c - 1):
+            put(done(u) + 1, h_quantize, u - 1, HALF * pair, HALF * (pair + 1))
+        put(done(u) + 1, h_quantize, u)
+        for pair in pairs(c - 1):
+            put(base + 4 + pair, unit_passes, u - 2, pair_tiles(pair))
+        put(end, vector_weave, u + 1)
+        for pair in pairs(c - 1):
+            put(end - 1 + pair, unit_passes, u - 1, pair_tiles(pair))
+        put(end, store_pair, c - 1, 0)
+        put(end, unit_passes, u, (0, 1))
+        put(end, vector_weave, u + 2)
+        put(end, h_quantize, u + 1)
+        put(end, unit_passes, u + 1, (0, 1))
+        put(end, weave, nc.vector.tensor_copy, u + 3, 0, P)
+        put(end, weave, nc.scalar.copy, u + 3, P, 2 * P)
+        put(end, h_quantize, u + 2)
+        put(end, unit_passes, u + 2, (0, 1))
+        for j in range(CHUNKS[c]):
+            put(end, h_quantize, u + 3, j * P, (j + 1) * P)
+            put(end, unit_passes, u + 3, (j,))
+        put(end, store_pair, c - 1, 1)
+        for j in range(CHUNKS[c]):
+            put(end, store_last, j)
 
         for k, (u, t) in enumerate(slots):
-            fill_bank(u, t)
+            scalar_bank(u, t)
             for work_fn, args in behind.get(k, []):
                 work_fn(*args)

@@ -170,26 +170,26 @@ def tile_spn_w4_kernel(tc, x_bytes, x_scale, w0_words, w0_scales, w1_words, w1_s
                 nc.scalar.activation(out=h_planes[u][:, t, :n], in_=bank[:, i, :], func=RELU, bias=bias_h[:, u % G, t : t + 1])
 
         def vector_bank(u, half, tag):
-            bank = psum.tile([P, 2, HALF], F32, name="zv", tag=tag, bufs=1)
+            bank = psum.tile([P, T, P], F32, name="zv", tag=tag, bufs=1)
             z_kept[u, half] = bank
-            for e in range(2):
-                plane(u, 2 * half + e, scalar_tokens(u), bank[:, e, :])
+            for t in range(T):
+                plane(u, t, scalar_tokens(u) + P * half, bank[:, t, :])
 
         def vector_bank_out(u, half):
             if half == 0:
-                h_pairs[u] = work.tile([P, 2, HALF, 2], BF16, name="hpair", bufs=1, align_bytes=64)
+                h_pairs[u] = work.tile([P, HALF, T], BF16, name="hpair", bufs=1, align_bytes=64)
             nc.vector.tensor_tensor(
-                out=h_pairs[u][:, half],
-                in0=z_kept[u, half][:].rearrange("p e n -> p n e"),
-                in1=bias_h[:, u % G, 2 * half : 2 * half + 2].unsqueeze(1).to_broadcast([P, HALF, 2]),
+                out=h_pairs[u][:, P * half : P * (half + 1)],
+                in0=z_kept[u, half][:].rearrange("p t n -> p n t"),
+                in1=bias_h[:, u % G, :].unsqueeze(1).to_broadcast([P, P, T]),
                 op=ADD,
             )
 
         def pairs_relu(u):
             lo = scalar_tokens(u)
             nc.vector.tensor_scalar(
-                out=woven_tile(u)[:, T * lo : T * (lo + HALF)].rearrange("p (n h e) -> p n h e", h=2, e=2),
-                in0=h_pairs[u][:].rearrange("p h n e -> p n h e"),
+                out=woven_tile(u)[:, T * lo : T * (lo + HALF)],
+                in0=h_pairs[u][:].rearrange("p n t -> p (n t)"),
                 scalar1=0.0,
                 scalar2=None,
                 op0=MAX,

@@ -28,11 +28,13 @@ FLOPS = 2 * B * X * N + 2 * B * H * OS
 
 CHUNKS = (2, 4, 4, 4, 2)
 MAX_TOKENS = max(CHUNKS) * P
+PAIR = 2 * P
 PLANE_BANKS = 4
 POOL_TOKENS = (256, 512, 512, 352)
+VECTOR_UNITS = (3, 6)
 PLANE_PAD = 16
-VECTOR_UNITS = (3, 6,)
-HALF = MAX_TOKENS // 2
+X_SLOTS = 2
+WEAVE_SLOTS = 2
 
 
 def tile_spn_w4_kernel(tc, x_bytes, x_scale, w0_words, w0_scales, w1_words, w1_scales, biases, out):
@@ -78,10 +80,36 @@ def tile_spn_w4_kernel(tc, x_bytes, x_scale, w0_words, w0_scales, w1_words, w1_s
         def load_w0(n0, n1):
             nc.sync.dma_start(out=w0_raw[:, 2 * n0 : 2 * n1], in_=w0_words[0, :, 2 * n0 : 2 * n1])
 
-        x_wide, x_turned, x_woven, x_codes, x_scales = {}, {}, {}, {}, {}
-        h_planes, h_woven, h_codes, h_scales, sums, z_kept, h_pairs = {}, {}, {}, {}, {}, {}, {}
+        for j in range(CHUNKS[0]):
+            nc.sync.dma_start(out=x_raw[0][:, j, :], in_=x_view[:, j, :])
+        nc.sync.dma_start(out=xs_col[:], in_=x_scale.rearrange("o (p t) -> p (o t)", t=T))
+        load_w0(0, PASS)
+        load_x(1)
+        for q in range(4):
+            nc.sync.dma_start(
+                out=w0s_raw[32 * q : 32 * q + 4, :].bitcast(I32),
+                in_=w0_scales[0, 4 * q : 4 * q + 4, :].bitcast(I32),
+            )
+        load_x(2)
+        load_w0(PASS, 2 * PASS)
+        nc.sync.dma_start(out=bias_h[:], in_=biases[0:H].rearrange("(g p t) -> p g t", g=G, p=P, t=T))
+        load_w0(2 * PASS, H)
+        load_x(3)
+        load_x(4)
+        load_w0(H, N)
+        nc.sync.dma_start(out=w1[:], in_=w1_words.rearrange("g p n -> p g n"))
+        for q in range(4):
+            nc.sync.dma_start(
+                out=w1s[32 * q : 32 * q + 4].bitcast(I32),
+                in_=w1_scales[:, 4 * q : 4 * q + 4, :].rearrange("g r n -> r g n").bitcast(I32),
+            )
+        nc.sync.dma_start(out=bias_o[:], in_=biases[H:N].partition_broadcast(P))
 
-        def permute_words(g0, g1, copy=nc.vector.tensor_copy):
+        x_wide, x_turned, x_woven, x_codes, x_scales = {}, {}, {}, {}, {}
+        h_planes, h_woven, h_codes, h_scales, sums, z_banks, z_woven = {}, {}, {}, {}, {}, {}, {}
+
+
+        def permute_words(g0, g1, copy):
             cols = slice(2 * PASS * g0, 2 * PASS * g1)
             copy(
                 out=w0_perm[:, cols].bitcast(U16).rearrange("p (g t m) -> p g t m", t=T, m=P),
@@ -95,6 +123,7 @@ def tile_spn_w4_kernel(tc, x_bytes, x_scale, w0_words, w0_scales, w1_words, w1_s
                 in_=w0s_raw[:, cols].rearrange("p (g m t) -> p g t m", t=T, m=P),
             )
 
+
         def x_cast(c, j0, count, cast):
             wide = keep.tile([P, count, X], BF16, name="xv%d_%d" % (c, j0), align_bytes=64)
             for jj in range(count):
@@ -104,7 +133,7 @@ def tile_spn_w4_kernel(tc, x_bytes, x_scale, w0_words, w0_scales, w1_words, w1_s
                 in_=x_raw[c][:, j0 : j0 + count, :].rearrange("p j k -> p (j k)").bitcast(FP8),
             )
 
-        def scalar_activation_cast(out, in_):
+        def scalar_first_cast(out, in_):
             nc.scalar.activation(out=out[:, :P], in_=in_[:, :P], func=COPY)
             nc.scalar.copy(out=out[:, P:], in_=in_[:, P:])
 
@@ -113,8 +142,8 @@ def tile_spn_w4_kernel(tc, x_bytes, x_scale, w0_words, w0_scales, w1_words, w1_s
             x_turned[c, j0] = bank
             for jj in range(count):
                 words = x_wide[c, j0 + jj].bitcast(F32)
-                for u in range(2):
-                    nc.tensor.transpose(bank[:, u, jj, :], words[:, u : X // 2 : 2], ident[:])
+                for a in range(2):
+                    nc.tensor.transpose(bank[:, a, jj, :], words[:, a : X // 2 : 2], ident[:])
 
         def x_scale_out(c, j0, count):
             if (c, j0) == (1, 0):
@@ -123,20 +152,20 @@ def tile_spn_w4_kernel(tc, x_bytes, x_scale, w0_words, w0_scales, w1_words, w1_s
                 x_woven[c, j0] = work.tile([P, T * MAX_TOKENS], BF16, name="xg", bufs=2, align_bytes=64)
             else:
                 x_woven[c, j0] = x_woven[c, 0]
-            halves = x_turned[c, j0][:].rearrange("p u j r -> p (u j r)").bitcast(BF16)
+            values = x_turned[c, j0][:].rearrange("p a j r -> p (a j r)").bitcast(BF16)
             nc.vector.tensor_tensor(
-                out=x_woven[c, j0][:, T * P * j0 : T * P * (j0 + count)].rearrange("p (r u e) -> p r u e", u=2, e=2),
-                in0=halves.rearrange("p (u r e) -> p r u e", u=2, e=2),
-                in1=xs_col[:].rearrange("p (o u e) -> p o u e", o=1, u=2).to_broadcast([P, count * P, 2, 2]),
+                out=x_woven[c, j0][:, T * P * j0 : T * P * (j0 + count)].rearrange("p (r a e) -> p r a e", a=2, e=2),
+                in0=values.rearrange("p (a r e) -> p r a e", a=2, e=2),
+                in1=xs_col[:].rearrange("p (o a e) -> p o a e", o=1, a=2).to_broadcast([P, count * P, 2, 2]),
                 op=MULT,
             )
 
-        def x_quantize(c, lo=0, hi=None):
-            hi = CHUNKS[c] * P if hi is None else hi
+        def x_quantize(c, lo, hi):
             if lo == 0:
                 x_codes[c] = work.tile([P, MAX_TOKENS], U32, name="xq", bufs=n_chunks, align_bytes=64)
                 x_scales[c] = work.tile([P, MAX_TOKENS], U8, name="xqs", bufs=n_chunks, align_bytes=64)
             nc.vector.quantize_mx(out=x_codes[c][:, lo:hi].bitcast(FP8X4), scales=x_scales[c][:, lo:hi], in_=x_woven[c, lo // P][:, T * lo : T * hi])
+
 
         def plane(u, t, lo, z):
             c, g = divmod(u, G)
@@ -153,15 +182,15 @@ def tile_spn_w4_kernel(tc, x_bytes, x_scale, w0_words, w0_scales, w1_words, w1_s
             )
 
         def scalar_tokens(u):
-            return tokens(u) - HALF if u in VECTOR_UNITS else tokens(u)
+            return tokens(u) - PAIR if u in VECTOR_UNITS else tokens(u)
 
-        def per_bank(u):
+        def planes_per_bank(u):
             return MAX_TOKENS // scalar_tokens(u) if u else 1
 
         def scalar_bank(u, t0):
-            n, count = scalar_tokens(u), per_bank(u)
+            n, count = scalar_tokens(u), planes_per_bank(u)
             if t0 == 0:
-                h_planes[u] = work.tile([P, T, MAX_TOKENS + PLANE_PAD], BF16, name="hp", bufs=6, align_bytes=64)
+                h_planes[u] = work.tile([P, T, MAX_TOKENS + PLANE_PAD], BF16, name="hp", bufs=n_units - 1, align_bytes=64)
             bank = psum.tile([P, count, n], F32, name="z", bufs=PLANE_BANKS)
             for i in range(count):
                 plane(u, t0 + i, 0, bank[:, i, :])
@@ -169,30 +198,20 @@ def tile_spn_w4_kernel(tc, x_bytes, x_scale, w0_words, w0_scales, w1_words, w1_s
                 t = t0 + i
                 nc.scalar.activation(out=h_planes[u][:, t, :n], in_=bank[:, i, :], func=RELU, bias=bias_h[:, u % G, t : t + 1])
 
-        def vector_bank(u, half, tag):
+        def vector_bank(u, i, tag):
             bank = psum.tile([P, T, P], F32, name="zv", tag=tag, bufs=1)
-            z_kept[u, half] = bank
+            z_banks[u, i] = bank
             for t in range(T):
-                plane(u, t, scalar_tokens(u) + P * half, bank[:, t, :])
+                plane(u, t, scalar_tokens(u) + P * i, bank[:, t, :])
 
-        def vector_bank_out(u, half):
-            if half == 0:
-                h_pairs[u] = work.tile([P, HALF, T], BF16, name="hpair", bufs=1, align_bytes=64)
+        def vector_bank_out(u, i):
+            if i == 0:
+                z_woven[u] = work.tile([P, PAIR, T], BF16, name="zg", bufs=len(VECTOR_UNITS), align_bytes=64)
             nc.vector.tensor_tensor(
-                out=h_pairs[u][:, P * half : P * (half + 1)],
-                in0=z_kept[u, half][:].rearrange("p t n -> p n t"),
+                out=z_woven[u][:, P * i : P * (i + 1)],
+                in0=z_banks[u, i][:].rearrange("p t n -> p n t"),
                 in1=bias_h[:, u % G, :].unsqueeze(1).to_broadcast([P, P, T]),
                 op=ADD,
-            )
-
-        def pairs_relu(u):
-            lo = scalar_tokens(u)
-            nc.vector.tensor_scalar(
-                out=woven_tile(u)[:, T * lo : T * (lo + HALF)],
-                in0=h_pairs[u][:].rearrange("p n t -> p (n t)"),
-                scalar1=0.0,
-                scalar2=None,
-                op0=MAX,
             )
 
         def woven_tile(u):
@@ -208,10 +227,17 @@ def tile_spn_w4_kernel(tc, x_bytes, x_scale, w0_words, w0_scales, w1_words, w1_s
             )
 
         def vector_weave(u):
+            n = scalar_tokens(u)
             if u in VECTOR_UNITS:
-                pairs_relu(u)
-            if scalar_tokens(u):
-                weave(nc.vector.tensor_copy, u, 0, scalar_tokens(u))
+                nc.vector.tensor_scalar(
+                    out=woven_tile(u)[:, T * n : T * (n + PAIR)],
+                    in0=z_woven[u][:].rearrange("p n t -> p (n t)"),
+                    scalar1=0.0,
+                    scalar2=None,
+                    op0=MAX,
+                )
+            if n:
+                weave(nc.vector.tensor_copy, u, 0, n)
 
         def pool_weave(u, lo, hi):
             nc.gpsimd.tensor_scalar(
@@ -223,18 +249,22 @@ def tile_spn_w4_kernel(tc, x_bytes, x_scale, w0_words, w0_scales, w1_words, w1_s
                 op1=ADD,
             )
 
-        def h_quantize(u, lo=0, hi=None):
-            hi = tokens(u) if hi is None else hi
-            if u not in h_codes:
-                h_codes[u] = work.tile([P, MAX_TOKENS], U32, name="hq", bufs=2 * G, align_bytes=64)
-                h_scales[u] = work.tile([P, MAX_TOKENS], U8, name="hqs", bufs=2 * G, align_bytes=64)
+        def h_quantize_part(u, lo, hi):
+            if lo == 0:
+                h_codes[u] = work.tile([P, MAX_TOKENS], U32, name="hq", bufs=n_units, align_bytes=64)
+                h_scales[u] = work.tile([P, MAX_TOKENS], U8, name="hqs", bufs=n_units, align_bytes=64)
             nc.vector.quantize_mx(out=h_codes[u][:, lo:hi].bitcast(FP8X4), scales=h_scales[u][:, lo:hi], in_=h_woven[u][:, T * lo : T * hi])
 
-        def out_pass(c, j, codes, scales, w, w_scales, start, stop):
-            per_bank = 1 if c == last else 2
-            bank, place = divmod(j, per_bank)
-            if start and place == 0:
-                sums[c, bank] = psum.tile([P, per_bank, OS], F32, name="o", tag=("x%d" if c == last else "o%d") % bank, bufs=1)
+        def h_quantize(u):
+            h_quantize_part(u, 0, tokens(u))
+
+
+        def out_pass(c, j, codes, scales, w, w_scales, opens, closes):
+            tiles_per_bank = 1 if c == last else 2
+            bank, place = divmod(j, tiles_per_bank)
+            if opens and place == 0:
+                tag = ("x%d" if c == last else "o%d") % bank
+                sums[c, bank] = psum.tile([P, tiles_per_bank, OS], F32, name="o", tag=tag, bufs=1)
             cols = slice(j * P, (j + 1) * P)
             nc.tensor.matmul_mx(
                 out=sums[c, bank][:, place, :],
@@ -242,8 +272,8 @@ def tile_spn_w4_kernel(tc, x_bytes, x_scale, w0_words, w0_scales, w1_words, w1_s
                 lhsT_scale=scales[:, cols],
                 rhs=w.bitcast(FP4X4),
                 rhs_scale=w_scales,
-                start=start and place == 0,
-                stop=stop and place == per_bank - 1,
+                start=opens and place == 0,
+                stop=closes and place == tiles_per_bank - 1,
             )
 
         def slice_passes(c, tiles):
@@ -256,67 +286,47 @@ def tile_spn_w4_kernel(tc, x_bytes, x_scale, w0_words, w0_scales, w1_words, w1_s
                 out_pass(c, j, h_codes[u], h_scales[u], w1[:, g, :], w1s[:, g, :], False, g == G - 1)
 
         def store_pair(c, pair):
-            res = work.tile([P, 2, OS], F32, name="res", bufs=4)
+            res = work.tile([P, 2, OS], F32, name="res", bufs=sum(CHUNKS[:last]) // 2)
             nc.vector.tensor_tensor(out=res[:], in0=sums[c, pair][:], in1=bias_o[:].unsqueeze(1).to_broadcast([P, 2, OS]), op=ADD)
             j0 = first_tile[c] + 2 * pair
             nc.sync.dma_start(out=out_view[:, j0 : j0 + 2, :], in_=res[:])
 
         def store_last(j):
-            res = work.tile([P, OS], F32, name="tail_res", bufs=2)
+            res = work.tile([P, OS], F32, name="tail_res", bufs=CHUNKS[last])
             nc.vector.tensor_tensor(out=res[:], in0=sums[last, j][:, 0, :], in1=bias_o[:], op=ADD)
             nc.sync.dma_start(out=out_view[:, first_tile[last] + j, :], in_=res[:])
 
-        load_x(0)
-        nc.sync.dma_start(out=xs_col[:], in_=x_scale.rearrange("o (p t) -> p (o t)", t=T))
-        load_w0(0, PASS)
-        load_x(1)
-        for q in range(4):
-            nc.sync.dma_start(
-                out=w0s_raw[32 * q : 32 * q + 4, :].bitcast(I32),
-                in_=w0_scales[0, 4 * q : 4 * q + 4, :].bitcast(I32),
-            )
-        load_x(2)
-        load_w0(PASS, 2 * PASS)
-        nc.sync.dma_start(out=bias_h[:], in_=biases[0:H].rearrange("(g p t) -> p g t", g=G, p=P, t=T))
         x_cast(0, 0, 1, nc.vector.tensor_copy)
-        x_cast(0, 1, 1, scalar_activation_cast)
-        load_w0(2 * PASS, H)
-        load_x(3)
-        load_x(4)
-        load_w0(H, N)
-        nc.sync.dma_start(out=w1[:], in_=w1_words.rearrange("g p n -> p g n"))
-        for q in range(4):
-            nc.sync.dma_start(
-                out=w1s[32 * q : 32 * q + 4].bitcast(I32),
-                in_=w1_scales[:, 4 * q : 4 * q + 4, :].rearrange("g r n -> r g n").bitcast(I32),
-            )
-        nc.sync.dma_start(out=bias_o[:], in_=biases[H:N].partition_broadcast(P))
-
+        x_cast(0, 1, 1, scalar_first_cast)
         x_transpose(0, 0, 1, "o0")
         x_transpose(0, 1, 1, "o1")
         x_cast(1, 0, 2, nc.scalar.copy)
         x_cast(1, 2, 2, nc.scalar.copy)
         x_cast(2, 0, 4, nc.scalar.copy)
-
-        permute_words(0, 1)
+        permute_words(0, 1, nc.vector.tensor_copy)
         x_transpose(1, 0, 2, "x0")
         x_transpose(1, 2, 2, "x1")
         for j in range(CHUNKS[0]):
             x_scale_out(0, j, 1)
         permute_scales(0, 1)
-        x_quantize(0)
+        x_quantize(0, 0, PAIR)
         permute_scales(1, 2)
         permute_words(1, 2, nc.scalar.copy)
         x_scale_out(1, 0, 2)
         permute_scales(2, G)
-        permute_words(2, 3)
-        x_quantize(1, 0, 2 * P)
-        permute_words(3, G)
+        permute_words(2, 3, nc.vector.tensor_copy)
+        x_quantize(1, 0, PAIR)
+        permute_words(3, G, nc.vector.tensor_copy)
 
+        slots = [(u, t) for u in range(n_units) if scalar_tokens(u) for t in range(0, T, planes_per_bank(u))]
+        end = len(slots) - 1
         behind = {}
 
         def put(k, work_fn, *args):
             behind.setdefault(k, []).append((work_fn, args))
+
+        def done(u):
+            return max(k for k, slot in enumerate(slots) if slot[0] <= u)
 
         def pairs(c):
             return range(CHUNKS[c] // 2)
@@ -324,46 +334,36 @@ def tile_spn_w4_kernel(tc, x_bytes, x_scale, w0_words, w0_scales, w1_words, w1_s
         def pair_tiles(pair):
             return (2 * pair, 2 * pair + 1)
 
-        slots = [(u, t) for u in range(n_units) if scalar_tokens(u) for t in range(0, T, per_bank(u))]
-
-        def done(u):
-            return max(k for k, slot in enumerate(slots) if slot[0] <= u)
-
-        end = len(slots) - 1
-
-        k = done(0)
-        put(k, pool_weave, 0, 0, tokens(0))
-        put(k, x_scale_out, 1, 2, 2)
-        k = done(2) - 1
-        for half in range(2):
-            put(k, vector_bank, 3, half, "o%d" % half)
-        put(k, vector_bank_out, 3, 0)
-        put(k, x_quantize, 1, HALF, 2 * HALF)
-        put(k, vector_bank_out, 3, 1)
-        put(k, h_quantize, 0)
+        put(done(0), pool_weave, 0, 0, POOL_TOKENS[0])
+        put(done(0), x_scale_out, 1, 2, 2)
         k = done(2)
+        for i in range(2):
+            put(k - 1, vector_bank, 3, i, "o%d" % i)
+        put(k - 1, vector_bank_out, 3, 0)
+        put(k - 1, x_quantize, 1, PAIR, 2 * PAIR)
+        put(k - 1, vector_bank_out, 3, 1)
+        put(k - 1, h_quantize, 0)
         put(k, vector_weave, 1)
         put(k, vector_weave, 2)
         put(k, h_quantize, 1)
-
-
         put(k, vector_weave, 3)
         put(k, h_quantize, 2)
         put(k, h_quantize, 3)
-        put(done(2) + 0, x_transpose, 2, 0, 2, "x0")
-        put(done(2) + 3, x_transpose, 2, 2, 2, "x1")
-        put(done(2) + 4, slice_passes, 0, (0, 1))
-        put(done(2) + 5, unit_passes, 0, (0, 1))
-        put(done(2) + 6, unit_passes, 1, (0, 1))
-
+        put(k, x_transpose, 2, 0, 2, "x0")
+        k += PLANE_BANKS - 1
+        put(k, x_transpose, 2, 2, 2, "x1")
+        put(k + 1, slice_passes, 0, pair_tiles(0))
+        put(k + 2, unit_passes, 0, pair_tiles(0))
+        put(k + 3, unit_passes, 1, pair_tiles(0))
         put(done(2), x_cast, 3, 0, 2, nc.scalar.copy)
-        put(done(4), x_cast, 3, 2, 2, nc.scalar.copy)
-        put(done(8), x_cast, 4, 0, 2, nc.scalar.copy)
+        put(done(G), x_cast, 3, 2, 2, nc.scalar.copy)
+        put(done(2 * G), x_cast, 4, 0, 2, nc.scalar.copy)
+
         for c in range(1, last):
             u = G * c
             n = tokens(u)
             cut = n - POOL_TOKENS[c]
-            window = done(u) + 4
+            window = done(u) + PLANE_BANKS
             put(window - 1, unit_passes, u - 2, range(CHUNKS[c - 1]))
             put(window, pool_weave, u, cut, n)
             for pair in pairs(c + 1):
@@ -372,61 +372,60 @@ def tile_spn_w4_kernel(tc, x_bytes, x_scale, w0_words, w0_scales, w1_words, w1_s
                 k = window + pair
                 put(k, unit_passes, u - 1, pair_tiles(pair))
                 put(k, store_pair, c - 1, pair)
-            if u + 2 in VECTOR_UNITS:
-                free = "x1" if c + 1 == last else "o1"
-                put(window - 0, vector_bank, u + 2, 0, free)
-                k = window + 2
+            shared = u + 2 in VECTOR_UNITS
+            if shared:
+                put(window, vector_bank, u + 2, 0, "o1")
+                k = window + X_SLOTS
                 put(k, vector_bank, u + 2, 1, "x0")
-                for half in range(2):
-                    put(k, vector_bank_out, u + 2, half)
+                for i in range(2):
+                    put(k, vector_bank_out, u + 2, i)
             if cut:
                 put(k, weave, nc.vector.tensor_copy, u, 0, cut)
-            put(k, x_quantize, c + 1)
+            put(k, x_quantize, c + 1, 0, tokens(u + G))
             put(k, h_quantize, u)
-            k = max(k, done(u + 1))
-            put(k, vector_weave, u + 1)
-            k = max(k, done(u + 2))
-            put(k, vector_weave, u + 2)
-            put(k, h_quantize, u + 1)
-            k = max(k, done(u + 3))
-            short = 2 if u + 2 in VECTOR_UNITS else 0
+            put(max(k, done(u + 1)), vector_weave, u + 1)
+            put(done(u + 2), vector_weave, u + 2)
+            put(done(u + 2), h_quantize, u + 1)
+            k = done(u + 3)
+            x_read = window + 2 * X_SLOTS
             if c + 1 < last:
                 put(k, vector_weave, u + 3)
                 put(k, h_quantize, u + 2)
                 put(k, h_quantize, u + 3)
                 for pair in pairs(c + 2):
-                    put(window + 5 + 2 * pair, x_transpose, c + 2, 2 * pair, 2, "x%d" % pair)
+                    put(x_read + 1 + 2 * pair, x_transpose, c + 2, 2 * pair, 2, "x%d" % pair)
             else:
                 put(k, h_quantize, u + 2)
                 put(k, vector_weave, u + 3)
+            opened = x_read + 2 + 1
             for pair in pairs(c):
-                put(window + 7 + pair, slice_passes, c, pair_tiles(pair))
-                put(window + 9 + pair, unit_passes, u, pair_tiles(pair))
-                put(window + 13 - short + pair, unit_passes, u + 1, pair_tiles(pair))
+                put(opened + pair, slice_passes, c, pair_tiles(pair))
+                put(opened + 2 + pair, unit_passes, u, pair_tiles(pair))
+                put(opened + 2 + 2 * WEAVE_SLOTS - (2 if shared else 0) + pair, unit_passes, u + 1, pair_tiles(pair))
 
         c, u = last, last * G
-        base = done(u - 1) + 1
-        put(base + 2, slice_passes, c, (0, 1))
-        put(done(u) + 1, vector_weave, u)
+        k = done(u)
+        put(k + 1, slice_passes, c, pair_tiles(0))
+        put(k + 1, vector_weave, u)
         for pair in pairs(c - 1):
-            put(done(u) + 1, h_quantize, u - 1, HALF * pair, HALF * (pair + 1))
-        put(done(u) + 1, h_quantize, u)
+            put(k + 1, h_quantize_part, u - 1, PAIR * pair, PAIR * (pair + 1))
+        put(k + 1, h_quantize, u)
         for pair in pairs(c - 1):
-            put(base + 4 + pair, unit_passes, u - 2, pair_tiles(pair))
+            put(k + 3 + pair, unit_passes, u - 2, pair_tiles(pair))
         put(end, vector_weave, u + 1)
         for pair in pairs(c - 1):
             put(end - 1 + pair, unit_passes, u - 1, pair_tiles(pair))
         put(end, store_pair, c - 1, 0)
-        put(end, unit_passes, u, (0, 1))
+        put(end, unit_passes, u, pair_tiles(0))
         put(end, vector_weave, u + 2)
         put(end, h_quantize, u + 1)
-        put(end, unit_passes, u + 1, (0, 1))
+        put(end, unit_passes, u + 1, pair_tiles(0))
         put(end, weave, nc.vector.tensor_copy, u + 3, 0, P)
-        put(end, weave, nc.scalar.copy, u + 3, P, 2 * P)
+        put(end, weave, nc.scalar.copy, u + 3, P, PAIR)
         put(end, h_quantize, u + 2)
-        put(end, unit_passes, u + 2, (0, 1))
+        put(end, unit_passes, u + 2, pair_tiles(0))
         for j in range(CHUNKS[c]):
-            put(end, h_quantize, u + 3, j * P, (j + 1) * P)
+            put(end, h_quantize_part, u + 3, j * P, (j + 1) * P)
             put(end, unit_passes, u + 3, (j,))
         put(end, store_pair, c - 1, 1)
         for j in range(CHUNKS[c]):

@@ -148,7 +148,9 @@ def tile_spn_w4_kernel(tc, x_bytes, x_scale, w0_words, w0_scales, w1_words, w1_s
         def x_scale_out(c, j0, count):
             if (c, j0) == (1, 0):
                 x_woven[c, j0] = work.tile([P, T * MAX_TOKENS], BF16, name="xg", tag="even", bufs=1, align_bytes=64)
-            elif j0 == 0 or c == 1:
+            elif (c, j0) == (1, 2):
+                x_woven[c, j0] = work.tile([P, T * MAX_TOKENS], BF16, name="xg", tag="one", bufs=1, align_bytes=64)
+            elif j0 == 0:
                 x_woven[c, j0] = work.tile([P, T * MAX_TOKENS], BF16, name="xg", bufs=2, align_bytes=64)
             else:
                 x_woven[c, j0] = x_woven[c, 0]
@@ -216,7 +218,7 @@ def tile_spn_w4_kernel(tc, x_bytes, x_scale, w0_words, w0_scales, w1_words, w1_s
 
         def woven_tile(u):
             if u not in h_woven:
-                tag, bufs = ("odd", 2) if u % 2 else ("even", 1)
+                tag, bufs = ("one", 1) if u == 1 else ("odd", 2) if u % 2 else ("even", 1)
                 h_woven[u] = work.tile([P, T * MAX_TOKENS], BF16, name="hg", tag=tag, bufs=bufs, align_bytes=64)
             return h_woven[u]
 
@@ -341,15 +343,17 @@ def tile_spn_w4_kernel(tc, x_bytes, x_scale, w0_words, w0_scales, w1_words, w1_s
             put(k - 1, vector_bank, 3, i, "o%d" % i)
         put(k - 1, vector_bank_out, 3, 0)
         put(k - 1, x_quantize, 1, PAIR, 2 * PAIR)
+        put(k - 1, pool_weave, 1, PAIR - 192, PAIR)
         put(k - 1, vector_bank_out, 3, 1)
-        put(k - 1, h_quantize, 0)
-        put(k, vector_weave, 1)
+        put(k, x_transpose, 2, 0, 2, "x0")
+        put(k, x_scale_out, 2, 0, 2)
+        put(k, h_quantize, 0)
+        put(k, weave, nc.vector.tensor_copy, 1, 0, PAIR - 192)
         put(k, vector_weave, 2)
-        put(k, h_quantize, 1)
         put(k, vector_weave, 3)
         put(k, h_quantize, 2)
+        put(k, h_quantize, 1)
         put(k, h_quantize, 3)
-        put(k, x_transpose, 2, 0, 2, "x0")
         k += PLANE_BANKS - 1
         put(k, x_transpose, 2, 2, 2, "x1")
         put(k + 1, slice_passes, 0, pair_tiles(0))
@@ -357,7 +361,7 @@ def tile_spn_w4_kernel(tc, x_bytes, x_scale, w0_words, w0_scales, w1_words, w1_s
         put(k + 3, unit_passes, 1, pair_tiles(0))
         put(done(2), x_cast, 3, 0, 2, nc.scalar.copy)
         put(done(G), x_cast, 3, 2, 2, nc.scalar.copy)
-        put(done(2 * G), x_cast, 4, 0, 2, nc.scalar.copy)
+        put(done(2 * G), x_cast, 4, 0, 1, nc.scalar.copy)
 
         for c in range(1, last):
             u = G * c
@@ -366,19 +370,17 @@ def tile_spn_w4_kernel(tc, x_bytes, x_scale, w0_words, w0_scales, w1_words, w1_s
             window = done(u) + PLANE_BANKS
             put(window - 1, unit_passes, u - 2, range(CHUNKS[c - 1]))
             put(window, pool_weave, u, cut, n)
-            for pair in pairs(c + 1):
+            for pair in pairs(c + 1)[0 if c > 1 else 1 :]:
                 put(window, x_scale_out, c + 1, 2 * pair, 2)
-            for pair in pairs(c - 1):
-                k = window + pair
-                put(k, unit_passes, u - 1, pair_tiles(pair))
-                put(k, store_pair, c - 1, pair)
             shared = u + 2 in VECTOR_UNITS
             if shared:
-                put(window, vector_bank, u + 2, 0, "o1")
-                k = window + X_SLOTS
-                put(k, vector_bank, u + 2, 1, "x0")
-                for i in range(2):
-                    put(k, vector_bank_out, u + 2, i)
+                for i, tag in enumerate(("o1", "x0")):
+                    put(window - 3 + i, vector_bank, u + 2, i, tag)
+                    put(window, vector_bank_out, u + 2, i)
+            for pair in pairs(c - 1):
+                k = window + pair + (0 if shared else 0)
+                put(k, unit_passes, u - 1, pair_tiles(pair))
+                put(k, store_pair, c - 1, pair)
             if cut:
                 put(k, weave, nc.vector.tensor_copy, u, 0, cut)
             put(k, x_quantize, c + 1, 0, tokens(u + G))
@@ -388,6 +390,8 @@ def tile_spn_w4_kernel(tc, x_bytes, x_scale, w0_words, w0_scales, w1_words, w1_s
             put(done(u + 2), h_quantize, u + 1)
             k = done(u + 3)
             x_read = window + 2 * X_SLOTS
+            if c == 1:
+                put(k, x_cast, 4, 1, 1, nc.vector.tensor_copy)
             if c + 1 < last:
                 put(k, vector_weave, u + 3)
                 put(k, h_quantize, u + 2)

@@ -30,8 +30,10 @@ CHUNKS = (2, 4, 4, 4, 2)
 MAX_TOKENS = max(CHUNKS) * P
 PAIR = 2 * P
 PLANE_BANKS = 4
-POOL_TOKENS = (256, 512, 512, 352)
-VECTOR_UNITS = (3, 6)
+POOL_TOKENS = (256, 512, 512, 384)
+POOL_MORE = (192, 0, 240, 0)
+SCALAR_TOKENS = 96
+VECTOR_UNITS = (3, 6, 10)
 PLANE_PAD = 16
 X_SLOTS = 2
 WEAVE_SLOTS = 2
@@ -343,12 +345,12 @@ def tile_spn_w4_kernel(tc, x_bytes, x_scale, w0_words, w0_scales, w1_words, w1_s
             put(k - 1, vector_bank, 3, i, "o%d" % i)
         put(k - 1, vector_bank_out, 3, 0)
         put(k - 1, x_quantize, 1, PAIR, 2 * PAIR)
-        put(k - 1, pool_weave, 1, PAIR - 192, PAIR)
+        put(k - 1, pool_weave, 1, PAIR - POOL_MORE[0], PAIR)
         put(k - 1, vector_bank_out, 3, 1)
         put(k, x_transpose, 2, 0, 2, "x0")
         put(k, x_scale_out, 2, 0, 2)
         put(k, h_quantize, 0)
-        put(k, weave, nc.vector.tensor_copy, 1, 0, PAIR - 192)
+        put(k, weave, nc.vector.tensor_copy, 1, 0, PAIR - POOL_MORE[0])
         put(k, vector_weave, 2)
         put(k, vector_weave, 3)
         put(k, h_quantize, 2)
@@ -361,7 +363,7 @@ def tile_spn_w4_kernel(tc, x_bytes, x_scale, w0_words, w0_scales, w1_words, w1_s
         put(k + 3, unit_passes, 1, pair_tiles(0))
         put(done(2), x_cast, 3, 0, 2, nc.scalar.copy)
         put(done(G), x_cast, 3, 2, 2, nc.scalar.copy)
-        put(done(2 * G), x_cast, 4, 0, 1, nc.scalar.copy)
+        put(done(2 * G), x_cast, 4, 0, 2, nc.scalar.copy)
 
         for c in range(1, last):
             u = G * c
@@ -370,42 +372,56 @@ def tile_spn_w4_kernel(tc, x_bytes, x_scale, w0_words, w0_scales, w1_words, w1_s
             window = done(u) + PLANE_BANKS
             put(window - 1, unit_passes, u - 2, range(CHUNKS[c - 1]))
             put(window, pool_weave, u, cut, n)
+            more = POOL_MORE[c]
+            if more:
+                put(window, pool_weave, u + 1, n - more, n)
             for pair in pairs(c + 1)[0 if c > 1 else 1 :]:
                 put(window, x_scale_out, c + 1, 2 * pair, 2)
-            shared = u + 2 in VECTOR_UNITS
-            if shared:
+            if c == 1:
                 for i, tag in enumerate(("o1", "x0")):
-                    put(window - 3 + i, vector_bank, u + 2, i, tag)
+                    put(done(u) + 1 + i, vector_bank, u + 2, i, tag)
                     put(window, vector_bank_out, u + 2, i)
             for pair in pairs(c - 1):
-                k = window + pair + (0 if shared else 0)
+                k = window + pair
                 put(k, unit_passes, u - 1, pair_tiles(pair))
                 put(k, store_pair, c - 1, pair)
+            if c == 2:
+                for i in range(2):
+                    k = window + X_SLOTS * (i + 1)
+                    put(k, vector_bank, u + 2, i, "x%d" % i)
+                    put(k, vector_bank_out, u + 2, i)
             if cut:
                 put(k, weave, nc.vector.tensor_copy, u, 0, cut)
             put(k, x_quantize, c + 1, 0, tokens(u + G))
             put(k, h_quantize, u)
-            put(max(k, done(u + 1)), vector_weave, u + 1)
-            put(done(u + 2), vector_weave, u + 2)
-            put(done(u + 2), h_quantize, u + 1)
+            if c == 2:
+                lo = n - more - SCALAR_TOKENS
+                put(k, weave, nc.vector.tensor_copy, u + 1, 0, lo)
+                put(done(u + 3), weave, nc.scalar.copy, u + 1, lo, n - more)
+                put(k, vector_weave, u + 2)
+                put(done(u + 3), h_quantize, u + 1)
+            else:
+                put(max(k, done(u + 1)), vector_weave, u + 1)
+                put(done(u + 2), vector_weave, u + 2)
+                put(done(u + 2), h_quantize, u + 1)
             k = done(u + 3)
             x_read = window + 2 * X_SLOTS
-            if c == 1:
-                put(k, x_cast, 4, 1, 1, nc.vector.tensor_copy)
             if c + 1 < last:
                 put(k, vector_weave, u + 3)
                 put(k, h_quantize, u + 2)
                 put(k, h_quantize, u + 3)
                 for pair in pairs(c + 2):
-                    put(x_read + 1 + 2 * pair, x_transpose, c + 2, 2 * pair, 2, "x%d" % pair)
+                    put(x_read + c + 2 * pair, x_transpose, c + 2, 2 * pair, 2, "x%d" % pair)
             else:
                 put(k, h_quantize, u + 2)
                 put(k, vector_weave, u + 3)
             opened = x_read + 2 + 1
+            ahead = (2, 1) if c == 2 else (0, 0)
+            short = 2 if u + 2 in VECTOR_UNITS else 0
             for pair in pairs(c):
-                put(opened + pair, slice_passes, c, pair_tiles(pair))
-                put(opened + 2 + pair, unit_passes, u, pair_tiles(pair))
-                put(opened + 2 + 2 * WEAVE_SLOTS - (2 if shared else 0) + pair, unit_passes, u + 1, pair_tiles(pair))
+                put(opened - ahead[0] + pair, slice_passes, c, pair_tiles(pair))
+                put(opened + 2 - ahead[1] + pair, unit_passes, u, pair_tiles(pair))
+                put(opened + 2 + 2 * WEAVE_SLOTS - short + pair, unit_passes, u + 1, pair_tiles(pair))
 
         c, u = last, last * G
         k = done(u)

@@ -26,39 +26,31 @@ G = H // PASS
 T = 4
 FLOPS = 2 * B * X * N + 2 * B * H * OS
 
-CHUNKS = (2, 4, 4, 4, 2)
-MAX_TOKENS = max(CHUNKS) * P
+TILES = 4
+CHUNK = TILES * P
+N_CHUNKS = B // CHUNK
 PAIR = 2 * P
 PLANE_BANKS = 4
-POOL_TOKENS = (256, 512, 512, 384)
-POOL_MORE = (192, 0, 240, 0)
-SCALAR_TOKENS = 96
-VECTOR_UNITS = (3, 6, 10)
 PLANE_PAD = 16
-X_SLOTS = 2
-WEAVE_SLOTS = 2
+POOL_TOKENS = (192, 456, 456, 96)
+SCALAR_TOKENS = (0, 408, 480, 32)
 
 
 def tile_spn_w4_kernel(tc, x_bytes, x_scale, w0_words, w0_scales, w1_words, w1_scales, biases, out):
     nc = tc.nc
-    n_chunks = len(CHUNKS)
-    last = n_chunks - 1
-    first_tile = [sum(CHUNKS[:c]) for c in range(n_chunks)]
-    n_units = n_chunks * G
+    last = N_CHUNKS - 1
     x_view = x_bytes.rearrange("(p j) k -> p j k", j=B // P)
     out_view = out.rearrange("(p j) n -> p j n", j=B // P)
 
-    def tokens(u):
-        return CHUNKS[u // G] * P
-
     with ExitStack() as ctx:
         keep = ctx.enter_context(tc.tile_pool(name="keep", bufs=1))
-        work = ctx.enter_context(tc.tile_pool(name="work", bufs=4))
         psum = ctx.enter_context(tc.psum_pool(name="psum", bufs=PLANE_BANKS))
         ctx.enter_context(tc.manual_schedule())
 
         ident = keep.tile([P, P], F32, name="ident")
-        w0_raw = keep.tile([P, 2 * N], U8, name="w0_raw", align_bytes=64)
+        w0_lo = keep.tile([P, 4 * PASS], U8, name="w0_lo", align_bytes=64)
+        w0_hi = keep.tile([P, 4 * PASS], U8, name="w0_hi", tag="gate0", align_bytes=64)
+        w0_out = keep.tile([P, 2 * OS], U8, name="w0_out", align_bytes=64)
         w0_perm = keep.tile([P, 2 * H], U8, name="w0_perm", align_bytes=64)
         w0s_raw = keep.tile([P, N], U8, name="w0s_raw", align_bytes=64)
         w0s_perm = keep.tile([P, H], U8, name="w0s_perm", align_bytes=64)
@@ -67,38 +59,38 @@ def tile_spn_w4_kernel(tc, x_bytes, x_scale, w0_words, w0_scales, w1_words, w1_s
         bias_h = keep.tile([P, G, T], BF16, name="bias_h")
         bias_o = keep.tile([P, OS], BF16, name="bias_o")
         xs_col = keep.tile([P, T], F32, name="xs_col")
-        x_raw = []
-        for c in range(n_chunks):
-            raw = keep.tile([P, CHUNKS[c], X], U8, name="xbytes%d" % c, align_bytes=64)
-            x_raw.append(raw)
+        x_raw = {}
 
         nc.vector.memset(w0s_raw[:].bitcast(I32), 0)
         nc.vector.memset(w1s[:].rearrange("p g n -> p (g n)").bitcast(I32), 0)
         make_identity(nc, ident[:])
 
-        def load_x(c):
-            nc.sync.dma_start(out=x_raw[c][:], in_=x_view[:, first_tile[c] : first_tile[c] + CHUNKS[c], :])
+        def load_x(j0, count):
+            raw = keep.tile([P, count, X], U8, name="xbytes%d" % j0, align_bytes=64)
+            for jj in range(count):
+                x_raw[j0 + jj] = (raw, jj)
+            nc.sync.dma_start(out=raw[:], in_=x_view[:, j0 : j0 + count, :])
 
-        def load_w0(n0, n1):
-            nc.sync.dma_start(out=w0_raw[:, 2 * n0 : 2 * n1], in_=w0_words[0, :, 2 * n0 : 2 * n1])
+        def load_w0(dst, n0, n1):
+            nc.sync.dma_start(out=dst, in_=w0_words[0, :, 2 * n0 : 2 * n1])
 
-        for j in range(CHUNKS[0]):
-            nc.sync.dma_start(out=x_raw[0][:, j, :], in_=x_view[:, j, :])
+        load_x(0, 1)
+        load_x(1, 1)
         nc.sync.dma_start(out=xs_col[:], in_=x_scale.rearrange("o (p t) -> p (o t)", t=T))
-        load_w0(0, PASS)
-        load_x(1)
+        load_w0(w0_lo[:, : 2 * PASS], 0, PASS)
+        load_x(2, 4)
         for q in range(4):
             nc.sync.dma_start(
                 out=w0s_raw[32 * q : 32 * q + 4, :].bitcast(I32),
                 in_=w0_scales[0, 4 * q : 4 * q + 4, :].bitcast(I32),
             )
-        load_x(2)
-        load_w0(PASS, 2 * PASS)
+        load_x(6, 4)
+        load_w0(w0_lo[:, 2 * PASS :], PASS, 2 * PASS)
         nc.sync.dma_start(out=bias_h[:], in_=biases[0:H].rearrange("(g p t) -> p g t", g=G, p=P, t=T))
-        load_w0(2 * PASS, H)
-        load_x(3)
-        load_x(4)
-        load_w0(H, N)
+        load_w0(w0_hi[:], 2 * PASS, H)
+        load_x(10, 4)
+        load_x(14, 2)
+        load_w0(w0_out[:], H, N)
         nc.sync.dma_start(out=w1[:], in_=w1_words.rearrange("g p n -> p g n"))
         for q in range(4):
             nc.sync.dma_start(
@@ -108,14 +100,12 @@ def tile_spn_w4_kernel(tc, x_bytes, x_scale, w0_words, w0_scales, w1_words, w1_s
         nc.sync.dma_start(out=bias_o[:], in_=biases[H:N].partition_broadcast(P))
 
         x_wide, x_turned, x_woven, x_codes, x_scales = {}, {}, {}, {}, {}
-        h_planes, h_woven, h_codes, h_scales, sums, z_banks, z_woven = {}, {}, {}, {}, {}, {}, {}
+        h_planes, h_woven, h_codes, h_scales, sums, z_banks, z_pairs = {}, {}, {}, {}, {}, {}, {}
 
-
-        def permute_words(g0, g1, copy):
-            cols = slice(2 * PASS * g0, 2 * PASS * g1)
+        def permute_words(raw, g0, g1, copy):
             copy(
-                out=w0_perm[:, cols].bitcast(U16).rearrange("p (g t m) -> p g t m", t=T, m=P),
-                in_=w0_raw[:, cols].bitcast(U16).rearrange("p (g m t) -> p g t m", t=T, m=P),
+                out=w0_perm[:, 2 * PASS * g0 : 2 * PASS * g1].bitcast(U16).rearrange("p (g t m) -> p g t m", t=T, m=P),
+                in_=raw.bitcast(U16).rearrange("p (g m t) -> p g t m", t=T, m=P),
             )
 
         def permute_scales(g0, g1):
@@ -125,14 +115,14 @@ def tile_spn_w4_kernel(tc, x_bytes, x_scale, w0_words, w0_scales, w1_words, w1_s
                 in_=w0s_raw[:, cols].rearrange("p (g m t) -> p g t m", t=T, m=P),
             )
 
-
         def x_cast(c, j0, count, cast):
             wide = keep.tile([P, count, X], BF16, name="xv%d_%d" % (c, j0), align_bytes=64)
             for jj in range(count):
                 x_wide[c, j0 + jj] = wide[:, jj, :]
+            raw, first = x_raw[TILES * c + j0]
             cast(
                 out=wide[:].rearrange("p j k -> p (j k)"),
-                in_=x_raw[c][:, j0 : j0 + count, :].rearrange("p j k -> p (j k)").bitcast(FP8),
+                in_=raw[:, first : first + count, :].rearrange("p j k -> p (j k)").bitcast(FP8),
             )
 
         def scalar_first_cast(out, in_):
@@ -148,17 +138,11 @@ def tile_spn_w4_kernel(tc, x_bytes, x_scale, w0_words, w0_scales, w1_words, w1_s
                     nc.tensor.transpose(bank[:, a, jj, :], words[:, a : X // 2 : 2], ident[:])
 
         def x_scale_out(c, j0, count):
-            if (c, j0) == (1, 0):
-                x_woven[c, j0] = work.tile([P, T * MAX_TOKENS], BF16, name="xg", tag="even", bufs=1, align_bytes=64)
-            elif (c, j0) == (1, 2):
-                x_woven[c, j0] = work.tile([P, T * MAX_TOKENS], BF16, name="xg", tag="one", bufs=1, align_bytes=64)
-            elif j0 == 0:
-                x_woven[c, j0] = work.tile([P, T * MAX_TOKENS], BF16, name="xg", bufs=2, align_bytes=64)
-            else:
-                x_woven[c, j0] = x_woven[c, 0]
+            if j0 == 0:
+                x_woven[c] = keep.tile([P, T * CHUNK], BF16, name="xg", tag="mid%d" % (c - 1), align_bytes=64)
             values = x_turned[c, j0][:].rearrange("p a j r -> p (a j r)").bitcast(BF16)
             nc.vector.tensor_tensor(
-                out=x_woven[c, j0][:, T * P * j0 : T * P * (j0 + count)].rearrange("p (r a e) -> p r a e", a=2, e=2),
+                out=x_woven[c][:, T * P * j0 : T * P * (j0 + count)].rearrange("p (r a e) -> p r a e", a=2, e=2),
                 in0=values.rearrange("p (a r e) -> p r a e", a=2, e=2),
                 in1=xs_col[:].rearrange("p (o a e) -> p o a e", o=1, a=2).to_broadcast([P, count * P, 2, 2]),
                 op=MULT,
@@ -166,13 +150,11 @@ def tile_spn_w4_kernel(tc, x_bytes, x_scale, w0_words, w0_scales, w1_words, w1_s
 
         def x_quantize(c, lo, hi):
             if lo == 0:
-                x_codes[c] = work.tile([P, MAX_TOKENS], U32, name="xq", bufs=n_chunks, align_bytes=64)
-                x_scales[c] = work.tile([P, MAX_TOKENS], U8, name="xqs", bufs=n_chunks, align_bytes=64)
-            nc.vector.quantize_mx(out=x_codes[c][:, lo:hi].bitcast(FP8X4), scales=x_scales[c][:, lo:hi], in_=x_woven[c, lo // P][:, T * lo : T * hi])
+                x_codes[c] = keep.tile([P, CHUNK], U32, name="xq%d" % c, align_bytes=64)
+                x_scales[c] = keep.tile([P, CHUNK], U8, name="xqs%d" % c, align_bytes=64)
+            nc.vector.quantize_mx(out=x_codes[c][:, lo:hi].bitcast(FP8X4), scales=x_scales[c][:, lo:hi], in_=x_woven[c][:, T * lo : T * hi])
 
-
-        def plane(u, t, lo, z):
-            c, g = divmod(u, G)
+        def plane(c, g, t, lo, z):
             m0 = PASS * g + P * t
             cols = slice(lo, lo + z.shape[1])
             nc.tensor.matmul_mx(
@@ -185,273 +167,280 @@ def tile_spn_w4_kernel(tc, x_bytes, x_scale, w0_words, w0_scales, w1_words, w1_s
                 stop=True,
             )
 
-        def scalar_tokens(u):
-            return tokens(u) - PAIR if u in VECTOR_UNITS else tokens(u)
+        def scalar_plane(c, g, t):
+            if t == 0:
+                h_planes[c, g] = keep.tile([P, T, CHUNK + PLANE_PAD], BF16, name="hp%d_%d" % (c, g), align_bytes=64)
+            bank = psum.tile([P, CHUNK], F32, name="z", bufs=PLANE_BANKS)
+            plane(c, g, t, 0, bank[:])
+            nc.scalar.activation(out=h_planes[c, g][:, t, :CHUNK], in_=bank[:], func=RELU, bias=bias_h[:, g, t : t + 1])
 
-        def planes_per_bank(u):
-            return MAX_TOKENS // scalar_tokens(u) if u else 1
-
-        def scalar_bank(u, t0):
-            n, count = scalar_tokens(u), planes_per_bank(u)
-            if t0 == 0:
-                h_planes[u] = work.tile([P, T, MAX_TOKENS + PLANE_PAD], BF16, name="hp", bufs=n_units - 1, align_bytes=64)
-            bank = psum.tile([P, count, n], F32, name="z", bufs=PLANE_BANKS)
+        def scalar_short_planes(g, pair, t0, count):
+            if (0, pair) not in h_planes:
+                h_planes[0, pair] = keep.tile([P, T, CHUNK + PLANE_PAD], BF16, name="hp0_%d" % pair, align_bytes=64)
+            bank = psum.tile([P, count, PAIR], F32, name="z", bufs=PLANE_BANKS)
             for i in range(count):
-                plane(u, t0 + i, 0, bank[:, i, :])
+                plane(0, g, t0 + i, PAIR * pair, bank[:, i, :])
             for i in range(count):
                 t = t0 + i
-                nc.scalar.activation(out=h_planes[u][:, t, :n], in_=bank[:, i, :], func=RELU, bias=bias_h[:, u % G, t : t + 1])
+                nc.scalar.activation(out=h_planes[0, pair][:, t, PAIR * g : PAIR * (g + 1)], in_=bank[:, i, :], func=RELU, bias=bias_h[:, g, t : t + 1])
 
-        def vector_bank(u, i, tag):
-            bank = psum.tile([P, T, P], F32, name="zv", tag=tag, bufs=1)
-            z_banks[u, i] = bank
-            for t in range(T):
-                plane(u, t, scalar_tokens(u) + P * i, bank[:, t, :])
+        def vector_bank(c, i, tag):
+            pair, a = divmod(i, 2)
+            bank = psum.tile([P, 2, PAIR], F32, name="zv", tag=tag, bufs=1)
+            z_banks[c, i] = bank
+            for e in range(2):
+                plane(c, G - 1, 2 * a + e, PAIR * pair, bank[:, e, :])
 
-        def vector_bank_out(u, i):
+        def vector_bank_out(c, i):
+            pair, a = divmod(i, 2)
             if i == 0:
-                z_woven[u] = work.tile([P, PAIR, T], BF16, name="zg", bufs=len(VECTOR_UNITS), align_bytes=64)
+                z_pairs[c] = keep.tile([P, 2, CHUNK + PLANE_PAD, 2], BF16, name="zg", bufs=2, align_bytes=64)
             nc.vector.tensor_tensor(
-                out=z_woven[u][:, P * i : P * (i + 1)],
-                in0=z_banks[u, i][:].rearrange("p t n -> p n t"),
-                in1=bias_h[:, u % G, :].unsqueeze(1).to_broadcast([P, P, T]),
+                out=z_pairs[c][:, a, PAIR * pair : PAIR * (pair + 1), :],
+                in0=z_banks[c, i][:].rearrange("p e n -> p n e"),
+                in1=bias_h[:, G - 1, 2 * a : 2 * a + 2].unsqueeze(1).to_broadcast([P, PAIR, 2]),
                 op=ADD,
             )
 
-        def woven_tile(u):
-            if u not in h_woven:
-                tag, bufs = ("one", 1) if u == 1 else ("odd", 2) if u % 2 else ("even", 1)
-                h_woven[u] = work.tile([P, T * MAX_TOKENS], BF16, name="hg", tag=tag, bufs=bufs, align_bytes=64)
-            return h_woven[u]
+        def woven_tile(c, g):
+            if (c, g) not in h_woven:
+                tag = "gate%d" % c if g == 0 else "gate%d" % (c + 1) if g == G - 1 else "mid%d" % c if g == 1 else "hg%d" % (c % 2)
+                h_woven[c, g] = keep.tile([P, T * CHUNK], BF16, name="hg", tag=tag, align_bytes=64)
+            return h_woven[c, g]
 
-        def weave(copy, u, lo, hi):
-            copy(
-                out=woven_tile(u)[:, T * lo : T * hi].rearrange("p (c i t) -> p c t i", t=T, i=4),
-                in_=h_planes[u][:, :, lo:hi].rearrange("p t (c i) -> p c t i", i=4),
+        def relu_join(c):
+            nc.vector.tensor_scalar(
+                out=woven_tile(c, G - 1)[:].rearrange("p (n a e) -> p n a e", a=2, e=2),
+                in0=z_pairs[c][:, :, :CHUNK, :].rearrange("p a n e -> p n a e"),
+                scalar1=0.0,
+                scalar2=None,
+                op0=MAX,
             )
 
-        def vector_weave(u):
-            n = scalar_tokens(u)
-            if u in VECTOR_UNITS:
-                nc.vector.tensor_scalar(
-                    out=woven_tile(u)[:, T * n : T * (n + PAIR)],
-                    in0=z_woven[u][:].rearrange("p n t -> p (n t)"),
-                    scalar1=0.0,
-                    scalar2=None,
-                    op0=MAX,
+        def weave(copy, c, g, lo, hi):
+            if hi > lo:
+                copy(
+                    out=woven_tile(c, g)[:, T * lo : T * hi].rearrange("p (c i t) -> p c t i", t=T, i=4),
+                    in_=h_planes[c, g][:, :, lo:hi].rearrange("p t (c i) -> p c t i", i=4),
                 )
-            if n:
-                weave(nc.vector.tensor_copy, u, 0, n)
 
-        def pool_weave(u, lo, hi):
-            nc.gpsimd.tensor_scalar(
-                out=woven_tile(u)[:, T * lo : T * hi].rearrange("p (n t) -> p n t", t=T),
-                in0=h_planes[u][:, :, lo:hi].rearrange("p t n -> p n t"),
-                scalar1=1.0,
-                scalar2=0.0,
-                op0=MULT,
-                op1=ADD,
-            )
+        def pool_weave(c, g, lo, hi):
+            if hi > lo:
+                nc.gpsimd.tensor_scalar(
+                    out=woven_tile(c, g)[:, T * lo : T * hi].rearrange("p (n t) -> p n t", t=T),
+                    in0=h_planes[c, g][:, :, lo:hi].rearrange("p t n -> p n t"),
+                    scalar1=1.0,
+                    scalar2=0.0,
+                    op0=MULT,
+                    op1=ADD,
+                )
 
-        def h_quantize_part(u, lo, hi):
-            if lo == 0:
-                h_codes[u] = work.tile([P, MAX_TOKENS], U32, name="hq", bufs=n_units, align_bytes=64)
-                h_scales[u] = work.tile([P, MAX_TOKENS], U8, name="hqs", bufs=n_units, align_bytes=64)
-            nc.vector.quantize_mx(out=h_codes[u][:, lo:hi].bitcast(FP8X4), scales=h_scales[u][:, lo:hi], in_=h_woven[u][:, T * lo : T * hi])
+        def share(c, g, lo, hi):
+            base = (g - 1) * CHUNK
+            return min(max(lo - base, 0), CHUNK), min(max(hi - base, 0), CHUNK)
 
-        def h_quantize(u):
-            h_quantize_part(u, 0, tokens(u))
+        def scalar_weave(c, g):
+            weave(nc.scalar.copy, c, g, *share(c, g, POOL_TOKENS[c], POOL_TOKENS[c] + SCALAR_TOKENS[c]))
 
+        def vector_weave(c, g):
+            weave(nc.vector.tensor_copy, c, g, *share(c, g, POOL_TOKENS[c] + SCALAR_TOKENS[c], 2 * CHUNK))
 
-        def out_pass(c, j, codes, scales, w, w_scales, opens, closes):
-            tiles_per_bank = 1 if c == last else 2
-            bank, place = divmod(j, tiles_per_bank)
+        def h_quantize(c, g, lo=0, hi=CHUNK):
+            if (c, g) not in h_codes:
+                h_codes[c, g] = keep.tile([P, CHUNK], U32, name="hq%d_%d" % (c, g), align_bytes=64)
+                h_scales[c, g] = keep.tile([P, CHUNK], U8, name="hqs%d_%d" % (c, g), align_bytes=64)
+            nc.vector.quantize_mx(out=h_codes[c, g][:, lo:hi].bitcast(FP8X4), scales=h_scales[c, g][:, lo:hi], in_=h_woven[c, g][:, T * lo : T * hi])
+
+        def sum_place(c, j):
+            if c == last and j >= 2:
+                return ("o1", "x0")[j - 2], 1, 0
+            return "o%d" % (j // 2), 2, j % 2
+
+        def out_pass(c, j, at, codes, scales, w, w_scales, opens, closes):
+            tag, count, place = sum_place(c, j)
             if opens and place == 0:
-                tag = ("x%d" if c == last else "o%d") % bank
-                sums[c, bank] = psum.tile([P, tiles_per_bank, OS], F32, name="o", tag=tag, bufs=1)
-            cols = slice(j * P, (j + 1) * P)
+                sums[c, tag] = psum.tile([P, count, OS], F32, name="o", tag=tag, bufs=1)
+            cols = slice(at * P, (at + 1) * P)
             nc.tensor.matmul_mx(
-                out=sums[c, bank][:, place, :],
+                out=sums[c, tag][:, place, :],
                 lhsT=codes[:, cols].bitcast(FP8X4),
                 lhsT_scale=scales[:, cols],
                 rhs=w.bitcast(FP4X4),
                 rhs_scale=w_scales,
                 start=opens and place == 0,
-                stop=closes and place == tiles_per_bank - 1,
+                stop=closes and place == count - 1,
             )
 
-        def slice_passes(c, tiles):
-            for j in tiles:
-                out_pass(c, j, x_codes[c], x_scales[c], w0_raw[:, 2 * H : 2 * N], w0s_raw[:, H:N], True, False)
+        def slice_passes(c, pair):
+            for j in (2 * pair, 2 * pair + 1):
+                out_pass(c, j, j, x_codes[c], x_scales[c], w0_out[:], w0s_raw[:, H:N], True, False)
 
-        def unit_passes(u, tiles):
-            c, g = divmod(u, G)
-            for j in tiles:
-                out_pass(c, j, h_codes[u], h_scales[u], w1[:, g, :], w1s[:, g, :], False, g == G - 1)
+        def unit_pass(c, g, j):
+            u, at = (j // 2, 2 * g + j % 2) if c == 0 and g < 2 else (g, j)
+            closing = 1 if c == last and j < 2 else 2
+            out_pass(c, j, at, h_codes[c, u], h_scales[c, u], w1[:, g, :], w1s[:, g, :], False, g == closing)
 
-        def store_pair(c, pair):
-            res = work.tile([P, 2, OS], F32, name="res", bufs=sum(CHUNKS[:last]) // 2)
-            nc.vector.tensor_tensor(out=res[:], in0=sums[c, pair][:], in1=bias_o[:].unsqueeze(1).to_broadcast([P, 2, OS]), op=ADD)
-            j0 = first_tile[c] + 2 * pair
-            nc.sync.dma_start(out=out_view[:, j0 : j0 + 2, :], in_=res[:])
+        def unit_passes(c, g, pair):
+            for j in (2 * pair, 2 * pair + 1):
+                unit_pass(c, g, j)
 
-        def store_last(j):
-            res = work.tile([P, OS], F32, name="tail_res", bufs=CHUNKS[last])
-            nc.vector.tensor_tensor(out=res[:], in0=sums[last, j][:, 0, :], in1=bias_o[:], op=ADD)
-            nc.sync.dma_start(out=out_view[:, first_tile[last] + j, :], in_=res[:])
+        def store(c, j0):
+            tag, count, place = sum_place(c, j0)
+            res = keep.tile([P, count, OS], F32, name="res", bufs=4)
+            nc.vector.tensor_tensor(out=res[:], in0=sums[c, tag][:], in1=bias_o[:].unsqueeze(1).to_broadcast([P, count, OS]), op=ADD)
+            nc.sync.dma_start(out=out_view[:, TILES * c + j0 : TILES * c + j0 + count, :], in_=res[:])
 
         x_cast(0, 0, 1, nc.vector.tensor_copy)
         x_cast(0, 1, 1, scalar_first_cast)
         x_transpose(0, 0, 1, "o0")
         x_transpose(0, 1, 1, "o1")
+        x_cast(0, 2, 2, nc.scalar.copy)
         x_cast(1, 0, 2, nc.scalar.copy)
         x_cast(1, 2, 2, nc.scalar.copy)
-        x_cast(2, 0, 4, nc.scalar.copy)
-        permute_words(0, 1, nc.vector.tensor_copy)
-        x_transpose(1, 0, 2, "x0")
-        x_transpose(1, 2, 2, "x1")
-        for j in range(CHUNKS[0]):
-            x_scale_out(0, j, 1)
+        x_cast(2, 0, 2, nc.scalar.copy)
+        permute_words(w0_lo[:, : 2 * PASS], 0, 1, nc.vector.tensor_copy)
+        x_transpose(0, 2, 2, "x0")
+        x_transpose(1, 0, 2, "x1")
+        x_scale_out(0, 0, 1)
+        x_scale_out(0, 1, 1)
         permute_scales(0, 1)
         x_quantize(0, 0, PAIR)
         permute_scales(1, 2)
-        permute_words(1, 2, nc.scalar.copy)
-        x_scale_out(1, 0, 2)
+        x_scale_out(0, 2, 2)
+        permute_words(w0_lo[:, 2 * PASS :], 1, 2, nc.scalar.copy)
+        permute_words(w0_hi[:], 2, G, nc.vector.tensor_copy)
+        x_quantize(0, PAIR, CHUNK)
         permute_scales(2, G)
-        permute_words(2, 3, nc.vector.tensor_copy)
-        x_quantize(1, 0, PAIR)
-        permute_words(3, G, nc.vector.tensor_copy)
-
-        slots = [(u, t) for u in range(n_units) if scalar_tokens(u) for t in range(0, T, planes_per_bank(u))]
-        end = len(slots) - 1
-        behind = {}
-
-        def put(k, work_fn, *args):
-            behind.setdefault(k, []).append((work_fn, args))
-
-        def done(u):
-            return max(k for k, slot in enumerate(slots) if slot[0] <= u)
-
-        def pairs(c):
-            return range(CHUNKS[c] // 2)
-
-        def pair_tiles(pair):
-            return (2 * pair, 2 * pair + 1)
-
-        put(done(0), pool_weave, 0, 0, POOL_TOKENS[0])
-        put(done(0), x_scale_out, 1, 2, 2)
-        k = done(2)
+        scalar_short_planes(0, 0, 0, 1)
+        scalar_short_planes(0, 0, 1, 1)
+        scalar_short_planes(0, 0, 2, 2)
+        pool_weave(0, 0, 0, PAIR)
+        for t in (0, 2):
+            scalar_short_planes(1, 0, t, 2)
+        pool_weave(0, 0, PAIR, CHUNK)
+        x_transpose(1, 2, 2, "o0")
+        x_scale_out(1, 0, 2)
+        x_scale_out(1, 2, 2)
+        tags = ("o1", "x0", "x1", "o0")
         for i in range(2):
-            put(k - 1, vector_bank, 3, i, "o%d" % i)
-        put(k - 1, vector_bank_out, 3, 0)
-        put(k - 1, x_quantize, 1, PAIR, 2 * PAIR)
-        put(k - 1, pool_weave, 1, PAIR - POOL_MORE[0], PAIR)
-        put(k - 1, vector_bank_out, 3, 1)
-        put(k, x_transpose, 2, 0, 2, "x0")
-        put(k, x_scale_out, 2, 0, 2)
-        put(k, h_quantize, 0)
-        put(k, weave, nc.vector.tensor_copy, 1, 0, PAIR - POOL_MORE[0])
-        put(k, vector_weave, 2)
-        put(k, vector_weave, 3)
-        put(k, h_quantize, 2)
-        put(k, h_quantize, 1)
-        put(k, h_quantize, 3)
-        k += PLANE_BANKS - 1
-        put(k, x_transpose, 2, 2, 2, "x1")
-        put(k + 1, slice_passes, 0, pair_tiles(0))
-        put(k + 2, unit_passes, 0, pair_tiles(0))
-        put(k + 3, unit_passes, 1, pair_tiles(0))
-        put(done(2), x_cast, 3, 0, 2, nc.scalar.copy)
-        put(done(G), x_cast, 3, 2, 2, nc.scalar.copy)
-        put(done(2 * G), x_cast, 4, 0, 2, nc.scalar.copy)
+            scalar_short_planes(0, 1, 2 * i, 2)
+            vector_bank(0, i, tags[i])
+        vector_bank_out(0, 0)
+        vector_bank_out(0, 1)
+        x_quantize(1, 0, CHUNK)
+        h_quantize(0, 0)
+        for i in range(2):
+            scalar_short_planes(1, 1, 2 * i, 2)
+            vector_bank(0, 2 + i, tags[2 + i])
+        pool_weave(0, 1, 0, POOL_TOKENS[0])
+        for i in range(2, 4):
+            vector_bank_out(0, i)
+        x_cast(2, 2, 2, nc.scalar.copy)
+        for t in range(T):
+            scalar_plane(0, 2, t)
+        x_cast(3, 0, 2, nc.scalar.copy)
 
-        for c in range(1, last):
-            u = G * c
-            n = tokens(u)
-            cut = n - POOL_TOKENS[c]
-            window = done(u) + PLANE_BANKS
-            put(window - 1, unit_passes, u - 2, range(CHUNKS[c - 1]))
-            put(window, pool_weave, u, cut, n)
-            more = POOL_MORE[c]
-            if more:
-                put(window, pool_weave, u + 1, n - more, n)
-            for pair in pairs(c + 1)[0 if c > 1 else 1 :]:
-                put(window, x_scale_out, c + 1, 2 * pair, 2)
-            if c == 1:
-                for i, tag in enumerate(("o1", "x0")):
-                    put(done(u) + 1 + i, vector_bank, u + 2, i, tag)
-                    put(window, vector_bank_out, u + 2, i)
-            for pair in pairs(c - 1):
-                k = window + pair
-                put(k, unit_passes, u - 1, pair_tiles(pair))
-                put(k, store_pair, c - 1, pair)
-            if c == 2:
-                for i in range(2):
-                    k = window + X_SLOTS * (i + 1)
-                    put(k, vector_bank, u + 2, i, "x%d" % i)
-                    put(k, vector_bank_out, u + 2, i)
-            if cut:
-                put(k, weave, nc.vector.tensor_copy, u, 0, cut)
-            put(k, x_quantize, c + 1, 0, tokens(u + G))
-            put(k, h_quantize, u)
-            if c == 2:
-                lo = n - more - SCALAR_TOKENS
-                put(k, weave, nc.vector.tensor_copy, u + 1, 0, lo)
-                put(done(u + 3), weave, nc.scalar.copy, u + 1, lo, n - more)
-                put(k, vector_weave, u + 2)
-                put(done(u + 3), h_quantize, u + 1)
+        for c in range(last):
+            d = c + 1
+            for pair in range(2):
+                if c == 0:
+                    scalar_plane(d, 0, pair)
+                if d < last:
+                    x_transpose(d + 1, 2 * pair, 2, "x%d" % pair)
+                else:
+                    vector_bank(d, pair, "x%d" % pair)
+            for pair in range(2):
+                if c == 0:
+                    scalar_plane(d, 0, 2 + pair)
+                slice_passes(c, pair)
+            if c == 0:
+                vector_weave(c, 1)
+                relu_join(c)
+                h_quantize(c, 1)
             else:
-                put(max(k, done(u + 1)), vector_weave, u + 1)
-                put(done(u + 2), vector_weave, u + 2)
-                put(done(u + 2), h_quantize, u + 1)
-            k = done(u + 3)
-            x_read = window + 2 * X_SLOTS
-            if c + 1 < last:
-                put(k, vector_weave, u + 3)
-                put(k, h_quantize, u + 2)
-                put(k, h_quantize, u + 3)
-                for pair in pairs(c + 2):
-                    put(x_read + c + 2 * pair, x_transpose, c + 2, 2 * pair, 2, "x%d" % pair)
+                h_quantize(c, 1)
+                relu_join(c)
+            vector_weave(c, 2)
+            h_quantize(c, 3)
+            h_quantize(c, 2)
+            pool_weave(d, 0, 0, CHUNK)
+            if d < last:
+                unit_passes(c, 0, 0)
+                scalar_plane(d, 1, 0)
+                unit_passes(c, 1, 0)
+                scalar_plane(d, 1, 1)
+                unit_passes(c, 0, 1)
+                scalar_plane(d, 1, 2)
+                unit_passes(c, 3, 0)
+                scalar_plane(d, 1, 3)
+                unit_passes(c, 2, 0)
+                scalar_plane(d, 2, 0)
+                unit_passes(c, 1, 1)
+                x_scale_out(d + 1, 0, 2)
+                scalar_plane(d, 2, 1)
+                unit_passes(c, 3, 1)
+                scalar_plane(d, 2, 2)
+                vector_bank(d, 0, "x0")
+                scalar_plane(d, 2, 3)
+                unit_passes(c, 2, 1)
+                x_scale_out(d + 1, 2, 2)
+                vector_bank(d, 1, "x1")
+                store(c, 0)
+                vector_bank(d, 2, "o0")
+                x_quantize(d + 1, 0, CHUNK)
+                h_quantize(d, 0)
+                pool_weave(d, 1, 0, POOL_TOKENS[d])
+                if d == 1:
+                    x_cast(3, 2, 2, nc.scalar.copy)
+                scalar_weave(d, 1)
+                scalar_weave(d, 2)
+                for t in range(T):
+                    scalar_plane(d + 1, 0, t)
+                store(c, 2)
+                vector_bank(d, 3, "o1")
+                for i in range(4):
+                    vector_bank_out(d, i)
             else:
-                put(k, h_quantize, u + 2)
-                put(k, vector_weave, u + 3)
-            opened = x_read + 2 + 1
-            ahead = (2, 1) if c == 2 else (0, 0)
-            short = 2 if u + 2 in VECTOR_UNITS else 0
-            for pair in pairs(c):
-                put(opened - ahead[0] + pair, slice_passes, c, pair_tiles(pair))
-                put(opened + 2 - ahead[1] + pair, unit_passes, u, pair_tiles(pair))
-                put(opened + 2 + 2 * WEAVE_SLOTS - short + pair, unit_passes, u + 1, pair_tiles(pair))
+                for g in range(2):
+                    for pair in range(2):
+                        unit_passes(c, g, pair)
+                    scalar_plane(d, 1, g)
+                scalar_plane(d, 1, 2)
+                unit_passes(c, 3, 0)
+                scalar_plane(d, 1, 3)
+                unit_passes(c, 2, 0)
+                vector_bank_out(d, 0)
+                vector_bank_out(d, 1)
+                store(c, 0)
+                for pair in range(2):
+                    vector_bank(d, 2 + pair, "x%d" % pair)
+                    scalar_plane(d, 2, pair)
+                    vector_bank_out(d, 2 + pair)
+                unit_passes(c, 3, 1)
+                unit_passes(c, 2, 1)
+                store(c, 2)
+                pool_weave(d, 1, 0, POOL_TOKENS[d])
 
-        c, u = last, last * G
-        k = done(u)
-        put(k + 1, slice_passes, c, pair_tiles(0))
-        put(k + 1, vector_weave, u)
-        for pair in pairs(c - 1):
-            put(k + 1, h_quantize_part, u - 1, PAIR * pair, PAIR * (pair + 1))
-        put(k + 1, h_quantize, u)
-        for pair in pairs(c - 1):
-            put(k + 3 + pair, unit_passes, u - 2, pair_tiles(pair))
-        put(end, vector_weave, u + 1)
-        for pair in pairs(c - 1):
-            put(end - 1 + pair, unit_passes, u - 1, pair_tiles(pair))
-        put(end, store_pair, c - 1, 0)
-        put(end, unit_passes, u, pair_tiles(0))
-        put(end, vector_weave, u + 2)
-        put(end, h_quantize, u + 1)
-        put(end, unit_passes, u + 1, pair_tiles(0))
-        put(end, weave, nc.vector.tensor_copy, u + 3, 0, P)
-        put(end, weave, nc.scalar.copy, u + 3, P, PAIR)
-        put(end, h_quantize, u + 2)
-        put(end, unit_passes, u + 2, pair_tiles(0))
-        for j in range(CHUNKS[c]):
-            put(end, h_quantize_part, u + 3, j * P, (j + 1) * P)
-            put(end, unit_passes, u + 3, (j,))
-        put(end, store_pair, c - 1, 1)
-        for j in range(CHUNKS[c]):
-            put(end, store_last, j)
-
-        for k, (u, t) in enumerate(slots):
-            scalar_bank(u, t)
-            for work_fn, args in behind.get(k, []):
-                work_fn(*args)
+        c = last
+        for pair in range(2):
+            scalar_plane(c, 2, 2 + pair)
+            slice_passes(c, pair)
+        scalar_weave(c, 1)
+        for pair in range(2):
+            weave(nc.scalar.copy, c, 2, PAIR * pair, PAIR * (pair + 1))
+        h_quantize(c, 0)
+        relu_join(c)
+        weave(nc.vector.tensor_copy, c, 1, POOL_TOKENS[c] + SCALAR_TOKENS[c], CHUNK)
+        for pair in range(2):
+            unit_passes(c, 0, pair)
+        for g in (3, 2, 1):
+            h_quantize(c, g, 0, PAIR)
+            unit_passes(c, g, 0)
+        for g in (3, 1):
+            h_quantize(c, g, PAIR, CHUNK)
+            unit_passes(c, g, 1)
+        for j in (2, 3):
+            h_quantize(c, 2, P * j, P * (j + 1))
+            unit_pass(c, 2, j)
+        for j in (0, 2, 3):
+            store(c, j)

@@ -32,8 +32,8 @@ N_CHUNKS = B // CHUNK
 PAIR = 2 * P
 PLANE_BANKS = 4
 PLANE_PAD = 16
-POOL_TOKENS = (192, 456, 456, 96)
-SCALAR_TOKENS = (0, 408, 480, 32)
+POOL_TOKENS = (192, 512, 456, 128)
+SCALAR_TOKENS = (0, 432, 432, 64)
 
 
 def tile_spn_w4_kernel(tc, x_bytes, x_scale, w0_words, w0_scales, w1_words, w1_scales, biases, out):
@@ -77,8 +77,8 @@ def tile_spn_w4_kernel(tc, x_bytes, x_scale, w0_words, w0_scales, w1_words, w1_s
         load_x(0, 1)
         load_x(1, 1)
         nc.sync.dma_start(out=xs_col[:], in_=x_scale.rearrange("o (p t) -> p (o t)", t=T))
-        load_w0(w0_lo[:, : 2 * PASS], 0, PASS)
         load_x(2, 4)
+        load_w0(w0_lo[:, : 2 * PASS], 0, PASS)
         for q in range(4):
             nc.sync.dma_start(
                 out=w0s_raw[32 * q : 32 * q + 4, :].bitcast(I32),
@@ -87,8 +87,8 @@ def tile_spn_w4_kernel(tc, x_bytes, x_scale, w0_words, w0_scales, w1_words, w1_s
         load_x(6, 4)
         load_w0(w0_lo[:, 2 * PASS :], PASS, 2 * PASS)
         nc.sync.dma_start(out=bias_h[:], in_=biases[0:H].rearrange("(g p t) -> p g t", g=G, p=P, t=T))
-        load_w0(w0_hi[:], 2 * PASS, H)
         load_x(10, 4)
+        load_w0(w0_hi[:], 2 * PASS, H)
         load_x(14, 2)
         load_w0(w0_out[:], H, N)
         nc.sync.dma_start(out=w1[:], in_=w1_words.rearrange("g p n -> p g n"))
@@ -204,7 +204,7 @@ def tile_spn_w4_kernel(tc, x_bytes, x_scale, w0_words, w0_scales, w1_words, w1_s
 
         def woven_tile(c, g):
             if (c, g) not in h_woven:
-                tag = "gate%d" % c if g == 0 else "gate%d" % (c + 1) if g == G - 1 else "mid%d" % c if g == 1 else "hg%d" % (c % 2)
+                tag = "gate%d" % c if g == 0 else "gate%d" % (c + 1) if g == 2 else "mid%d" % c if g == 1 else "hg%d" % (c % 2)
                 h_woven[c, g] = keep.tile([P, T * CHUNK], BF16, name="hg", tag=tag, align_bytes=64)
             return h_woven[c, g]
 
@@ -234,16 +234,6 @@ def tile_spn_w4_kernel(tc, x_bytes, x_scale, w0_words, w0_scales, w1_words, w1_s
                     op0=MULT,
                     op1=ADD,
                 )
-
-        def share(c, g, lo, hi):
-            base = (g - 1) * CHUNK
-            return min(max(lo - base, 0), CHUNK), min(max(hi - base, 0), CHUNK)
-
-        def scalar_weave(c, g):
-            weave(nc.scalar.copy, c, g, *share(c, g, POOL_TOKENS[c], POOL_TOKENS[c] + SCALAR_TOKENS[c]))
-
-        def vector_weave(c, g):
-            weave(nc.vector.tensor_copy, c, g, *share(c, g, POOL_TOKENS[c] + SCALAR_TOKENS[c], 2 * CHUNK))
 
         def h_quantize(c, g, lo=0, hi=CHUNK):
             if (c, g) not in h_codes:
@@ -277,8 +267,7 @@ def tile_spn_w4_kernel(tc, x_bytes, x_scale, w0_words, w0_scales, w1_words, w1_s
 
         def unit_pass(c, g, j):
             u, at = (j // 2, 2 * g + j % 2) if c == 0 and g < 2 else (g, j)
-            closing = 1 if c == last and j < 2 else 2
-            out_pass(c, j, at, h_codes[c, u], h_scales[c, u], w1[:, g, :], w1s[:, g, :], False, g == closing)
+            out_pass(c, j, at, h_codes[c, u], h_scales[c, u], w1[:, g, :], w1s[:, g, :], False, g == (2 if c == last else 3))
 
         def unit_passes(c, g, pair):
             for j in (2 * pair, 2 * pair + 1):
@@ -289,6 +278,9 @@ def tile_spn_w4_kernel(tc, x_bytes, x_scale, w0_words, w0_scales, w1_words, w1_s
             res = keep.tile([P, count, OS], F32, name="res", bufs=4)
             nc.vector.tensor_tensor(out=res[:], in0=sums[c, tag][:], in1=bias_o[:].unsqueeze(1).to_broadcast([P, count, OS]), op=ADD)
             nc.sync.dma_start(out=out_view[:, TILES * c + j0 : TILES * c + j0 + count, :], in_=res[:])
+
+        def x_bank(c, pair):
+            return "x%d" % ((c + pair) % 2)
 
         x_cast(0, 0, 1, nc.vector.tensor_copy)
         x_cast(0, 1, 1, scalar_first_cast)
@@ -308,6 +300,7 @@ def tile_spn_w4_kernel(tc, x_bytes, x_scale, w0_words, w0_scales, w1_words, w1_s
         permute_scales(1, 2)
         x_scale_out(0, 2, 2)
         permute_words(w0_lo[:, 2 * PASS :], 1, 2, nc.scalar.copy)
+        x_cast(2, 2, 2, nc.scalar.copy)
         permute_words(w0_hi[:], 2, G, nc.vector.tensor_copy)
         x_quantize(0, PAIR, CHUNK)
         permute_scales(2, G)
@@ -335,10 +328,10 @@ def tile_spn_w4_kernel(tc, x_bytes, x_scale, w0_words, w0_scales, w1_words, w1_s
         pool_weave(0, 1, 0, POOL_TOKENS[0])
         for i in range(2, 4):
             vector_bank_out(0, i)
-        x_cast(2, 2, 2, nc.scalar.copy)
         for t in range(T):
             scalar_plane(0, 2, t)
         x_cast(3, 0, 2, nc.scalar.copy)
+        weave(nc.scalar.copy, 0, 2, 0, SCALAR_TOKENS[0])
 
         for c in range(last):
             d = c + 1
@@ -346,23 +339,20 @@ def tile_spn_w4_kernel(tc, x_bytes, x_scale, w0_words, w0_scales, w1_words, w1_s
                 if c == 0:
                     scalar_plane(d, 0, pair)
                 if d < last:
-                    x_transpose(d + 1, 2 * pair, 2, "x%d" % pair)
+                    x_transpose(d + 1, 2 * pair, 2, x_bank(d + 1, pair))
                 else:
-                    vector_bank(d, pair, "x%d" % pair)
+                    vector_bank(d, pair, x_bank(d + 1, pair))
             for pair in range(2):
                 if c == 0:
                     scalar_plane(d, 0, 2 + pair)
                 slice_passes(c, pair)
             if c == 0:
-                vector_weave(c, 1)
-                relu_join(c)
-                h_quantize(c, 1)
-            else:
-                h_quantize(c, 1)
-                relu_join(c)
-            vector_weave(c, 2)
-            h_quantize(c, 3)
+                weave(nc.vector.tensor_copy, c, 1, POOL_TOKENS[c], CHUNK)
+            weave(nc.vector.tensor_copy, c, 2, SCALAR_TOKENS[c], CHUNK)
+            relu_join(c)
+            h_quantize(c, 1)
             h_quantize(c, 2)
+            h_quantize(c, 3)
             pool_weave(d, 0, 0, CHUNK)
             if d < last:
                 unit_passes(c, 0, 0)
@@ -371,20 +361,20 @@ def tile_spn_w4_kernel(tc, x_bytes, x_scale, w0_words, w0_scales, w1_words, w1_s
                 scalar_plane(d, 1, 1)
                 unit_passes(c, 0, 1)
                 scalar_plane(d, 1, 2)
-                unit_passes(c, 3, 0)
-                scalar_plane(d, 1, 3)
                 unit_passes(c, 2, 0)
+                scalar_plane(d, 1, 3)
+                unit_passes(c, 3, 0)
                 scalar_plane(d, 2, 0)
                 unit_passes(c, 1, 1)
                 x_scale_out(d + 1, 0, 2)
                 scalar_plane(d, 2, 1)
-                unit_passes(c, 3, 1)
-                scalar_plane(d, 2, 2)
-                vector_bank(d, 0, "x0")
-                scalar_plane(d, 2, 3)
                 unit_passes(c, 2, 1)
+                scalar_plane(d, 2, 2)
+                vector_bank(d, 0, x_bank(d + 1, 0))
+                scalar_plane(d, 2, 3)
+                unit_passes(c, 3, 1)
                 x_scale_out(d + 1, 2, 2)
-                vector_bank(d, 1, "x1")
+                vector_bank(d, 1, x_bank(d + 1, 1))
                 store(c, 0)
                 vector_bank(d, 2, "o0")
                 x_quantize(d + 1, 0, CHUNK)
@@ -392,48 +382,55 @@ def tile_spn_w4_kernel(tc, x_bytes, x_scale, w0_words, w0_scales, w1_words, w1_s
                 pool_weave(d, 1, 0, POOL_TOKENS[d])
                 if d == 1:
                     x_cast(3, 2, 2, nc.scalar.copy)
-                scalar_weave(d, 1)
-                scalar_weave(d, 2)
+                weave(nc.scalar.copy, d, 1, POOL_TOKENS[d], CHUNK)
+                weave(nc.scalar.copy, d, 2, 0, SCALAR_TOKENS[d])
+                vector_bank_out(d, 0)
                 for t in range(T):
+                    if t == 2:
+                        vector_bank(d, 3, x_bank(d + 1, 0))
                     scalar_plane(d + 1, 0, t)
-                store(c, 2)
-                vector_bank(d, 3, "o1")
-                for i in range(4):
+                for i in range(1, 4):
                     vector_bank_out(d, i)
+                store(c, 2)
             else:
-                for g in range(2):
-                    for pair in range(2):
-                        unit_passes(c, g, pair)
-                    scalar_plane(d, 1, g)
+                unit_passes(c, 0, 0)
+                unit_passes(c, 0, 1)
+                scalar_plane(d, 1, 0)
+                scalar_plane(d, 1, 1)
+                unit_passes(c, 1, 0)
+                unit_passes(c, 1, 1)
                 scalar_plane(d, 1, 2)
-                unit_passes(c, 3, 0)
-                scalar_plane(d, 1, 3)
                 unit_passes(c, 2, 0)
+                scalar_plane(d, 1, 3)
+                unit_passes(c, 3, 0)
                 vector_bank_out(d, 0)
                 vector_bank_out(d, 1)
                 store(c, 0)
                 for pair in range(2):
-                    vector_bank(d, 2 + pair, "x%d" % pair)
                     scalar_plane(d, 2, pair)
+                    vector_bank(d, 2 + pair, "x%d" % pair)
                     vector_bank_out(d, 2 + pair)
-                unit_passes(c, 3, 1)
                 unit_passes(c, 2, 1)
+                scalar_plane(d, 2, 2)
+                unit_passes(c, 3, 1)
+                scalar_plane(d, 2, 3)
                 store(c, 2)
                 pool_weave(d, 1, 0, POOL_TOKENS[d])
 
         c = last
         for pair in range(2):
-            scalar_plane(c, 2, 2 + pair)
             slice_passes(c, pair)
-        scalar_weave(c, 1)
-        for pair in range(2):
-            weave(nc.scalar.copy, c, 2, PAIR * pair, PAIR * (pair + 1))
+        weave(nc.scalar.copy, c, 1, PAIR - SCALAR_TOKENS[c], PAIR)
+        weave(nc.scalar.copy, c, 1, PAIR, CHUNK)
+        for j in (2, 3):
+            weave(nc.scalar.copy, c, 2, P * j, P * (j + 1))
         h_quantize(c, 0)
         relu_join(c)
-        weave(nc.vector.tensor_copy, c, 1, POOL_TOKENS[c] + SCALAR_TOKENS[c], CHUNK)
+        weave(nc.vector.tensor_copy, c, 1, POOL_TOKENS[c], PAIR - SCALAR_TOKENS[c])
+        weave(nc.vector.tensor_copy, c, 2, 0, PAIR)
         for pair in range(2):
             unit_passes(c, 0, pair)
-        for g in (3, 2, 1):
+        for g in (3, 1, 2):
             h_quantize(c, g, 0, PAIR)
             unit_passes(c, g, 0)
         for g in (3, 1):

@@ -33,7 +33,7 @@ PAIR = 2 * P
 PLANE_BANKS = 4
 PLANE_PAD = 16
 POOL_TOKENS = (192, 512, 456, 128)
-SCALAR_TOKENS = (0, 432, 432, 64)
+SCALAR_TOKENS = (0, 384, 384, 64)
 
 
 def tile_spn_w4_kernel(tc, x_bytes, x_scale, w0_words, w0_scales, w1_words, w1_scales, biases, out):
@@ -74,29 +74,26 @@ def tile_spn_w4_kernel(tc, x_bytes, x_scale, w0_words, w0_scales, w1_words, w1_s
         def load_w0(dst, n0, n1):
             nc.sync.dma_start(out=dst, in_=w0_words[0, :, 2 * n0 : 2 * n1])
 
+        def load_w0_scales(n0, n1):
+            for r in range(4):
+                nc.sync.dma_start(out=w0s_raw[r:P:32, n0:n1].bitcast(I32), in_=w0_scales[0, r:16:4, n0:n1].bitcast(I32))
+
         load_x(0, 1)
         load_x(1, 1)
         nc.sync.dma_start(out=xs_col[:], in_=x_scale.rearrange("o (p t) -> p (o t)", t=T))
-        load_x(2, 4)
+        load_x(2, 2)
         load_w0(w0_lo[:, : 2 * PASS], 0, PASS)
-        for q in range(4):
-            nc.sync.dma_start(
-                out=w0s_raw[32 * q : 32 * q + 4, :].bitcast(I32),
-                in_=w0_scales[0, 4 * q : 4 * q + 4, :].bitcast(I32),
-            )
-        load_x(6, 4)
+        load_x(4, 2)
         load_w0(w0_lo[:, 2 * PASS :], PASS, 2 * PASS)
+        load_w0_scales(0, N)
+        load_x(6, 4)
         nc.sync.dma_start(out=bias_h[:], in_=biases[0:H].rearrange("(g p t) -> p g t", g=G, p=P, t=T))
-        load_x(10, 4)
         load_w0(w0_hi[:], 2 * PASS, H)
-        load_x(14, 2)
+        load_x(10, 6)
         load_w0(w0_out[:], H, N)
         nc.sync.dma_start(out=w1[:], in_=w1_words.rearrange("g p n -> p g n"))
-        for q in range(4):
-            nc.sync.dma_start(
-                out=w1s[32 * q : 32 * q + 4].bitcast(I32),
-                in_=w1_scales[:, 4 * q : 4 * q + 4, :].rearrange("g r n -> r g n").bitcast(I32),
-            )
+        for r in range(4):
+            nc.sync.dma_start(out=w1s[r:P:32].bitcast(I32), in_=w1_scales[:, r:16:4, :].rearrange("g q n -> q g n").bitcast(I32))
         nc.sync.dma_start(out=bias_o[:], in_=biases[H:N].partition_broadcast(P))
 
         x_wide, x_turned, x_woven, x_codes, x_scales = {}, {}, {}, {}, {}
@@ -288,6 +285,7 @@ def tile_spn_w4_kernel(tc, x_bytes, x_scale, w0_words, w0_scales, w1_words, w1_s
         x_transpose(0, 1, 1, "o1")
         x_cast(0, 2, 2, nc.scalar.copy)
         x_cast(1, 0, 2, nc.scalar.copy)
+        permute_words(w0_lo[:, 2 * PASS :], 1, 2, nc.scalar.copy)
         x_cast(1, 2, 2, nc.scalar.copy)
         x_cast(2, 0, 2, nc.scalar.copy)
         permute_words(w0_lo[:, : 2 * PASS], 0, 1, nc.vector.tensor_copy)
@@ -299,8 +297,6 @@ def tile_spn_w4_kernel(tc, x_bytes, x_scale, w0_words, w0_scales, w1_words, w1_s
         x_quantize(0, 0, PAIR)
         permute_scales(1, 2)
         x_scale_out(0, 2, 2)
-        permute_words(w0_lo[:, 2 * PASS :], 1, 2, nc.scalar.copy)
-        x_cast(2, 2, 2, nc.scalar.copy)
         permute_words(w0_hi[:], 2, G, nc.vector.tensor_copy)
         x_quantize(0, PAIR, CHUNK)
         permute_scales(2, G)
@@ -328,6 +324,7 @@ def tile_spn_w4_kernel(tc, x_bytes, x_scale, w0_words, w0_scales, w1_words, w1_s
         pool_weave(0, 1, 0, POOL_TOKENS[0])
         for i in range(2, 4):
             vector_bank_out(0, i)
+        x_cast(2, 2, 2, nc.scalar.copy)
         for t in range(T):
             scalar_plane(0, 2, t)
         x_cast(3, 0, 2, nc.scalar.copy)
@@ -348,8 +345,8 @@ def tile_spn_w4_kernel(tc, x_bytes, x_scale, w0_words, w0_scales, w1_words, w1_s
                 slice_passes(c, pair)
             if c == 0:
                 weave(nc.vector.tensor_copy, c, 1, POOL_TOKENS[c], CHUNK)
-            weave(nc.vector.tensor_copy, c, 2, SCALAR_TOKENS[c], CHUNK)
             relu_join(c)
+            weave(nc.vector.tensor_copy, c, 2, SCALAR_TOKENS[c], CHUNK)
             h_quantize(c, 1)
             h_quantize(c, 2)
             h_quantize(c, 3)

@@ -33,7 +33,7 @@ PAIR = 2 * P
 PLANE_BANKS = 4
 PLANE_PAD = 16
 POOL_TOKENS = (192, 512, 456, 128)
-SCALAR_TOKENS = (0, 384, 384, 64)
+SCALAR_TOKENS = (96, 480, 480, 96)
 
 
 def tile_spn_w4_kernel(tc, x_bytes, x_scale, w0_words, w0_scales, w1_words, w1_scales, biases, out):

@@ -32,8 +32,8 @@ N_CHUNKS = B // CHUNK
 PAIR = 2 * P
 PLANE_BANKS = 4
 PLANE_PAD = 16
-POOL_TOKENS = (192, 512, 456, 128)
-SCALAR_TOKENS = (96, 480, 480, 96)
+POOL_TOKENS = (192, 512, 512, 128)
+SCALAR_TOKENS = (128, 512, 512, 128)
 
 
 def tile_spn_w4_kernel(tc, x_bytes, x_scale, w0_words, w0_scales, w1_words, w1_scales, biases, out):
@@ -164,22 +164,25 @@ def tile_spn_w4_kernel(tc, x_bytes, x_scale, w0_words, w0_scales, w1_words, w1_s
                 stop=True,
             )
 
+        def planes_view(c, g):
+            first = min(g, 1)
+            if (c, first) not in h_planes:
+                width = CHUNK * (1 + first) + PLANE_PAD
+                h_planes[c, first] = keep.tile([P, T, width], BF16, name="hp%d_%d" % (c, first), align_bytes=64)
+            return h_planes[c, first][:, :, CHUNK * (g - first) :]
+
         def scalar_plane(c, g, t):
-            if t == 0:
-                h_planes[c, g] = keep.tile([P, T, CHUNK + PLANE_PAD], BF16, name="hp%d_%d" % (c, g), align_bytes=64)
             bank = psum.tile([P, CHUNK], F32, name="z", bufs=PLANE_BANKS)
             plane(c, g, t, 0, bank[:])
-            nc.scalar.activation(out=h_planes[c, g][:, t, :CHUNK], in_=bank[:], func=RELU, bias=bias_h[:, g, t : t + 1])
+            nc.scalar.activation(out=planes_view(c, g)[:, t, :CHUNK], in_=bank[:], func=RELU, bias=bias_h[:, g, t : t + 1])
 
         def scalar_short_planes(g, pair, t0, count):
-            if (0, pair) not in h_planes:
-                h_planes[0, pair] = keep.tile([P, T, CHUNK + PLANE_PAD], BF16, name="hp0_%d" % pair, align_bytes=64)
             bank = psum.tile([P, count, PAIR], F32, name="z", bufs=PLANE_BANKS)
             for i in range(count):
                 plane(0, g, t0 + i, PAIR * pair, bank[:, i, :])
             for i in range(count):
                 t = t0 + i
-                nc.scalar.activation(out=h_planes[0, pair][:, t, PAIR * g : PAIR * (g + 1)], in_=bank[:, i, :], func=RELU, bias=bias_h[:, g, t : t + 1])
+                nc.scalar.activation(out=planes_view(0, pair)[:, t, PAIR * g : PAIR * (g + 1)], in_=bank[:, i, :], func=RELU, bias=bias_h[:, g, t : t + 1])
 
         def vector_bank(c, i, tag):
             pair, a = divmod(i, 2)
@@ -199,15 +202,16 @@ def tile_spn_w4_kernel(tc, x_bytes, x_scale, w0_words, w0_scales, w1_words, w1_s
                 op=ADD,
             )
 
-        def woven_tile(c, g):
-            if (c, g) not in h_woven:
-                tag = "gate%d" % c if g == 0 else "gate%d" % (c + 1) if g == 2 else "mid%d" % c if g == 1 else "hg%d" % (c % 2)
-                h_woven[c, g] = keep.tile([P, T * CHUNK], BF16, name="hg", tag=tag, align_bytes=64)
-            return h_woven[c, g]
+        def woven_view(c, g):
+            key = 1 if g == 2 else g
+            if (c, key) not in h_woven:
+                tag = "mid%d" % c if key == 1 else "gate%d" % (c + 1 if key else c)
+                h_woven[c, key] = keep.tile([P, T * CHUNK * (2 if key == 1 else 1)], BF16, name="hg", tag=tag, align_bytes=64)
+            return h_woven[c, key][:, T * CHUNK * (g - key) :]
 
         def relu_join(c):
             nc.vector.tensor_scalar(
-                out=woven_tile(c, G - 1)[:].rearrange("p (n a e) -> p n a e", a=2, e=2),
+                out=woven_view(c, G - 1).rearrange("p (n a e) -> p n a e", a=2, e=2),
                 in0=z_pairs[c][:, :, :CHUNK, :].rearrange("p a n e -> p n a e"),
                 scalar1=0.0,
                 scalar2=None,
@@ -217,15 +221,15 @@ def tile_spn_w4_kernel(tc, x_bytes, x_scale, w0_words, w0_scales, w1_words, w1_s
         def weave(copy, c, g, lo, hi):
             if hi > lo:
                 copy(
-                    out=woven_tile(c, g)[:, T * lo : T * hi].rearrange("p (c i t) -> p c t i", t=T, i=4),
-                    in_=h_planes[c, g][:, :, lo:hi].rearrange("p t (c i) -> p c t i", i=4),
+                    out=woven_view(c, g)[:, T * lo : T * hi].rearrange("p (c i t) -> p c t i", t=T, i=4),
+                    in_=planes_view(c, g)[:, :, lo:hi].rearrange("p t (c i) -> p c t i", i=4),
                 )
 
         def pool_weave(c, g, lo, hi):
             if hi > lo:
                 nc.gpsimd.tensor_scalar(
-                    out=woven_tile(c, g)[:, T * lo : T * hi].rearrange("p (n t) -> p n t", t=T),
-                    in0=h_planes[c, g][:, :, lo:hi].rearrange("p t n -> p n t"),
+                    out=woven_view(c, g)[:, T * lo : T * hi].rearrange("p (n t) -> p n t", t=T),
+                    in0=planes_view(c, g)[:, :, lo:hi].rearrange("p t n -> p n t"),
                     scalar1=1.0,
                     scalar2=0.0,
                     op0=MULT,
@@ -236,12 +240,18 @@ def tile_spn_w4_kernel(tc, x_bytes, x_scale, w0_words, w0_scales, w1_words, w1_s
             if (c, g) not in h_codes:
                 h_codes[c, g] = keep.tile([P, CHUNK], U32, name="hq%d_%d" % (c, g), align_bytes=64)
                 h_scales[c, g] = keep.tile([P, CHUNK], U8, name="hqs%d_%d" % (c, g), align_bytes=64)
-            nc.vector.quantize_mx(out=h_codes[c, g][:, lo:hi].bitcast(FP8X4), scales=h_scales[c, g][:, lo:hi], in_=h_woven[c, g][:, T * lo : T * hi])
+            nc.vector.quantize_mx(out=h_codes[c, g][:, lo:hi].bitcast(FP8X4), scales=h_scales[c, g][:, lo:hi], in_=woven_view(c, g)[:, T * lo : T * hi])
+
+        def side_banks(c):
+            ring = ("x1", "o1", "o0")
+            k = 2 * (c - 1)
+            return ("x0", ring[k % 3], ring[(k + 1) % 3], ring[(k + 2) % 3])
 
         def sum_place(c, j):
+            banks = side_banks(c + 1)
             if c == last and j >= 2:
-                return ("o1", "x0")[j - 2], 1, 0
-            return "o%d" % (j // 2), 2, j % 2
+                return (banks[3], banks[0])[j - 2], 1, 0
+            return banks[2 + j // 2], 2, j % 2
 
         def out_pass(c, j, at, codes, scales, w, w_scales, opens, closes):
             tag, count, place = sum_place(c, j)
@@ -264,7 +274,7 @@ def tile_spn_w4_kernel(tc, x_bytes, x_scale, w0_words, w0_scales, w1_words, w1_s
 
         def unit_pass(c, g, j):
             u, at = (j // 2, 2 * g + j % 2) if c == 0 and g < 2 else (g, j)
-            out_pass(c, j, at, h_codes[c, u], h_scales[c, u], w1[:, g, :], w1s[:, g, :], False, g == (2 if c == last else 3))
+            out_pass(c, j, at, h_codes[c, u], h_scales[c, u], w1[:, g, :], w1s[:, g, :], False, g == 2)
 
         def unit_passes(c, g, pair):
             for j in (2 * pair, 2 * pair + 1):
@@ -275,9 +285,6 @@ def tile_spn_w4_kernel(tc, x_bytes, x_scale, w0_words, w0_scales, w1_words, w1_s
             res = keep.tile([P, count, OS], F32, name="res", bufs=4)
             nc.vector.tensor_tensor(out=res[:], in0=sums[c, tag][:], in1=bias_o[:].unsqueeze(1).to_broadcast([P, count, OS]), op=ADD)
             nc.sync.dma_start(out=out_view[:, TILES * c + j0 : TILES * c + j0 + count, :], in_=res[:])
-
-        def x_bank(c, pair):
-            return "x%d" % ((c + pair) % 2)
 
         x_cast(0, 0, 1, nc.vector.tensor_copy)
         x_cast(0, 1, 1, scalar_first_cast)
@@ -328,89 +335,92 @@ def tile_spn_w4_kernel(tc, x_bytes, x_scale, w0_words, w0_scales, w1_words, w1_s
         for t in range(T):
             scalar_plane(0, 2, t)
         x_cast(3, 0, 2, nc.scalar.copy)
-        weave(nc.scalar.copy, 0, 2, 0, SCALAR_TOKENS[0])
+        weave(nc.scalar.copy, 0, 1, 2 * CHUNK - SCALAR_TOKENS[0], 2 * CHUNK)
 
         for c in range(last):
             d = c + 1
-            for pair in range(2):
-                if c == 0:
-                    scalar_plane(d, 0, pair)
-                if d < last:
-                    x_transpose(d + 1, 2 * pair, 2, x_bank(d + 1, pair))
-                else:
-                    vector_bank(d, pair, x_bank(d + 1, pair))
-            for pair in range(2):
-                if c == 0:
-                    scalar_plane(d, 0, 2 + pair)
-                slice_passes(c, pair)
+            banks = side_banks(d)
             if c == 0:
                 weave(nc.vector.tensor_copy, c, 1, POOL_TOKENS[c], CHUNK)
             relu_join(c)
-            weave(nc.vector.tensor_copy, c, 2, SCALAR_TOKENS[c], CHUNK)
+            weave(nc.vector.tensor_copy, c, 1, max(POOL_TOKENS[c], CHUNK), 2 * CHUNK - SCALAR_TOKENS[c])
             h_quantize(c, 1)
-            h_quantize(c, 2)
             h_quantize(c, 3)
-            pool_weave(d, 0, 0, CHUNK)
-            if d < last:
+            h_quantize(c, 2)
+            if c == 0:
+                scalar_plane(d, 0, 0)
+                slice_passes(c, 0)
+                scalar_plane(d, 0, 1)
+                x_transpose(d + 1, 0, 2, banks[0])
+                scalar_plane(d, 0, 2)
+                x_transpose(d + 1, 2, 2, banks[1])
+                scalar_plane(d, 0, 3)
                 unit_passes(c, 0, 0)
                 scalar_plane(d, 1, 0)
-                unit_passes(c, 1, 0)
+                slice_passes(c, 1)
                 scalar_plane(d, 1, 1)
                 unit_passes(c, 0, 1)
-                scalar_plane(d, 1, 2)
-                unit_passes(c, 2, 0)
-                scalar_plane(d, 1, 3)
-                unit_passes(c, 3, 0)
+            else:
+                for pair in range(2):
+                    if d < last:
+                        x_transpose(d + 1, 2 * pair, 2, banks[pair])
+                    else:
+                        vector_bank(d, pair, banks[pair])
+                    scalar_plane(d, 1, pair)
+            pool_weave(d, 0, 0, CHUNK)
+            if d < last:
+                for t, g in ((2, 1), (3, 3)):
+                    scalar_plane(d, 1, t)
+                    unit_passes(c, g, 0)
                 scalar_plane(d, 2, 0)
-                unit_passes(c, 1, 1)
+                unit_passes(c, 2, 0)
                 x_scale_out(d + 1, 0, 2)
                 scalar_plane(d, 2, 1)
-                unit_passes(c, 2, 1)
+                vector_bank(d, 0, banks[0])
                 scalar_plane(d, 2, 2)
-                vector_bank(d, 0, x_bank(d + 1, 0))
+                unit_passes(c, 1, 1)
                 scalar_plane(d, 2, 3)
-                unit_passes(c, 3, 1)
                 x_scale_out(d + 1, 2, 2)
-                vector_bank(d, 1, x_bank(d + 1, 1))
+                vector_bank(d, 1, banks[1])
+                unit_passes(c, 3, 1)
                 store(c, 0)
-                vector_bank(d, 2, "o0")
+                vector_bank(d, 2, banks[2])
+                unit_passes(c, 2, 1)
                 x_quantize(d + 1, 0, CHUNK)
                 h_quantize(d, 0)
                 pool_weave(d, 1, 0, POOL_TOKENS[d])
                 if d == 1:
                     x_cast(3, 2, 2, nc.scalar.copy)
                 weave(nc.scalar.copy, d, 1, POOL_TOKENS[d], CHUNK)
-                weave(nc.scalar.copy, d, 2, 0, SCALAR_TOKENS[d])
+                weave(nc.scalar.copy, d, 1, 2 * CHUNK - SCALAR_TOKENS[d], 2 * CHUNK)
                 vector_bank_out(d, 0)
-                for t in range(T):
-                    if t == 2:
-                        vector_bank(d, 3, x_bank(d + 1, 0))
-                    scalar_plane(d + 1, 0, t)
+                scalar_plane(d + 1, 0, 0)
+                scalar_plane(d + 1, 0, 1)
+                vector_bank(d, 3, banks[0])
                 for i in range(1, 4):
                     vector_bank_out(d, i)
                 store(c, 2)
+                for pair in range(2):
+                    scalar_plane(d + 1, 0, 2 + pair)
+                    slice_passes(d, pair)
+                    unit_passes(d, 0, pair)
             else:
-                unit_passes(c, 0, 0)
-                unit_passes(c, 0, 1)
-                scalar_plane(d, 1, 0)
-                scalar_plane(d, 1, 1)
                 unit_passes(c, 1, 0)
-                unit_passes(c, 1, 1)
                 scalar_plane(d, 1, 2)
-                unit_passes(c, 2, 0)
+                unit_passes(c, 1, 1)
                 scalar_plane(d, 1, 3)
                 unit_passes(c, 3, 0)
+                unit_passes(c, 2, 0)
                 vector_bank_out(d, 0)
                 vector_bank_out(d, 1)
                 store(c, 0)
                 for pair in range(2):
                     scalar_plane(d, 2, pair)
-                    vector_bank(d, 2 + pair, "x%d" % pair)
+                    vector_bank(d, 2 + pair, banks[pair])
                     vector_bank_out(d, 2 + pair)
-                unit_passes(c, 2, 1)
-                scalar_plane(d, 2, 2)
-                unit_passes(c, 3, 1)
-                scalar_plane(d, 2, 3)
+                for pair in range(2):
+                    unit_passes(c, 3 - pair, 1)
+                    scalar_plane(d, 2, 2 + pair)
                 store(c, 2)
                 pool_weave(d, 1, 0, POOL_TOKENS[d])
 

@@ -314,6 +314,7 @@ def tile_spn_w4_kernel(tc, x_bytes, x_scale, w0_words, w0_scales, w1_words, w1_s
         for t in (0, 2):
             scalar_short_planes(1, 0, t, 2)
         pool_weave(0, 0, PAIR, CHUNK)
+        x_cast(2, 2, 2, nc.scalar.copy)
         x_transpose(1, 2, 2, "o0")
         x_scale_out(1, 0, 2)
         x_scale_out(1, 2, 2)
@@ -331,7 +332,6 @@ def tile_spn_w4_kernel(tc, x_bytes, x_scale, w0_words, w0_scales, w1_words, w1_s
         pool_weave(0, 1, 0, POOL_TOKENS[0])
         for i in range(2, 4):
             vector_bank_out(0, i)
-        x_cast(2, 2, 2, nc.scalar.copy)
         for t in range(T):
             scalar_plane(0, 2, t)
         x_cast(3, 0, 2, nc.scalar.copy)

@@ -185,20 +185,18 @@ def tile_spn_w4_kernel(tc, x_bytes, x_scale, w0_words, w0_scales, w1_words, w1_s
                 nc.scalar.activation(out=planes_view(0, pair)[:, t, PAIR * g : PAIR * (g + 1)], in_=bank[:, i, :], func=RELU, bias=bias_h[:, g, t : t + 1])
 
         def vector_bank(c, i, tag):
-            pair, a = divmod(i, 2)
-            bank = psum.tile([P, 2, PAIR], F32, name="zv", tag=tag, bufs=1)
+            bank = psum.tile([P, T, P], F32, name="zv", tag=tag, bufs=1)
             z_banks[c, i] = bank
-            for e in range(2):
-                plane(c, G - 1, 2 * a + e, PAIR * pair, bank[:, e, :])
+            for t in range(T):
+                plane(c, G - 1, t, P * i, bank[:, t, :])
 
         def vector_bank_out(c, i):
-            pair, a = divmod(i, 2)
             if i == 0:
-                z_pairs[c] = keep.tile([P, 2, CHUNK + PLANE_PAD, 2], BF16, name="zg", bufs=2, align_bytes=64)
+                z_pairs[c] = keep.tile([P, CHUNK, T], BF16, name="zg", bufs=2, align_bytes=64)
             nc.vector.tensor_tensor(
-                out=z_pairs[c][:, a, PAIR * pair : PAIR * (pair + 1), :],
-                in0=z_banks[c, i][:].rearrange("p e n -> p n e"),
-                in1=bias_h[:, G - 1, 2 * a : 2 * a + 2].unsqueeze(1).to_broadcast([P, PAIR, 2]),
+                out=z_pairs[c][:, P * i : P * (i + 1), :],
+                in0=z_banks[c, i][:].rearrange("p t n -> p n t"),
+                in1=bias_h[:, G - 1, :].unsqueeze(1).to_broadcast([P, P, T]),
                 op=ADD,
             )
 
@@ -211,8 +209,8 @@ def tile_spn_w4_kernel(tc, x_bytes, x_scale, w0_words, w0_scales, w1_words, w1_s
 
         def relu_join(c):
             nc.vector.tensor_scalar(
-                out=woven_view(c, G - 1).rearrange("p (n a e) -> p n a e", a=2, e=2),
-                in0=z_pairs[c][:, :, :CHUNK, :].rearrange("p a n e -> p n a e"),
+                out=woven_view(c, G - 1),
+                in0=z_pairs[c][:].rearrange("p n t -> p (n t)"),
                 scalar1=0.0,
                 scalar2=None,
                 op0=MAX,

@@ -32,8 +32,8 @@ N_CHUNKS = B // CHUNK
 PAIR = 2 * P
 PLANE_BANKS = 4
 PLANE_PAD = 16
-POOL_TOKENS = (192, 512, 512, 128)
-SCALAR_TOKENS = (128, 512, 512, 128)
+POOL_TOKENS = (192, 512, 512, 96)
+SCALAR_TOKENS = (96, 512, 512)
 
 
 def tile_spn_w4_kernel(tc, x_bytes, x_scale, w0_words, w0_scales, w1_words, w1_scales, biases, out):
@@ -203,7 +203,7 @@ def tile_spn_w4_kernel(tc, x_bytes, x_scale, w0_words, w0_scales, w1_words, w1_s
         def woven_view(c, g):
             key = 1 if g == 2 else g
             if (c, key) not in h_woven:
-                tag = "mid%d" % c if key == 1 else "gate%d" % (c + 1 if key else c)
+                tag = ("mid%d" if c < last else "gate%d") % c if key == 1 else "gate%d" % (c + 1 if key else c)
                 h_woven[c, key] = keep.tile([P, T * CHUNK * (2 if key == 1 else 1)], BF16, name="hg", tag=tag, align_bytes=64)
             return h_woven[c, key][:, T * CHUNK * (g - key) :]
 
@@ -405,33 +405,35 @@ def tile_spn_w4_kernel(tc, x_bytes, x_scale, w0_words, w0_scales, w1_words, w1_s
             else:
                 unit_passes(c, 1, 0)
                 scalar_plane(d, 1, 2)
-                unit_passes(c, 1, 1)
                 scalar_plane(d, 1, 3)
                 unit_passes(c, 3, 0)
                 unit_passes(c, 2, 0)
                 vector_bank_out(d, 0)
                 vector_bank_out(d, 1)
                 store(c, 0)
-                for pair in range(2):
-                    scalar_plane(d, 2, pair)
-                    vector_bank(d, 2 + pair, banks[pair])
-                    vector_bank_out(d, 2 + pair)
-                for pair in range(2):
-                    unit_passes(c, 3 - pair, 1)
-                    scalar_plane(d, 2, 2 + pair)
-                store(c, 2)
-                pool_weave(d, 1, 0, POOL_TOKENS[d])
+                scalar_plane(d, 2, 0)
+                vector_bank(d, 2, banks[0])
+                vector_bank_out(d, 2)
+                scalar_plane(d, 2, 1)
+                vector_bank(d, 3, banks[1])
+                vector_bank_out(d, 3)
+                scalar_plane(d, 2, 2)
+                scalar_plane(d, 2, 3)
+                unit_passes(c, 1, 1)
+                unit_passes(c, 3, 1)
+                unit_passes(c, 2, 1)
 
         c = last
         for pair in range(2):
             slice_passes(c, pair)
-        weave(nc.scalar.copy, c, 1, PAIR - SCALAR_TOKENS[c], PAIR)
+        h_quantize(c, 0)
+        pool_weave(c, 1, 0, POOL_TOKENS[c])
+        weave(nc.scalar.copy, c, 1, POOL_TOKENS[c], PAIR)
         weave(nc.scalar.copy, c, 1, PAIR, CHUNK)
         for j in (2, 3):
             weave(nc.scalar.copy, c, 2, P * j, P * (j + 1))
-        h_quantize(c, 0)
         relu_join(c)
-        weave(nc.vector.tensor_copy, c, 1, POOL_TOKENS[c], PAIR - SCALAR_TOKENS[c])
+        store(c - 1, 2)
         weave(nc.vector.tensor_copy, c, 2, 0, PAIR)
         for pair in range(2):
             unit_passes(c, 0, pair)

@@ -247,8 +247,8 @@ def tile_spn_w4_kernel(tc, x_bytes, x_scale, w0_words, w0_scales, w1_words, w1_s
 
         def sum_place(c, j):
             banks = side_banks(c + 1)
-            if c == last and j >= 2:
-                return (banks[3], banks[0])[j - 2], 1, 0
+            if c == last:
+                return (banks[2], banks[1], banks[3], banks[0])[j], 1, 0
             return banks[2 + j // 2], 2, j % 2
 
         def out_pass(c, j, at, codes, scales, w, w_scales, opens, closes):
@@ -266,13 +266,16 @@ def tile_spn_w4_kernel(tc, x_bytes, x_scale, w0_words, w0_scales, w1_words, w1_s
                 stop=closes and place == count - 1,
             )
 
+        def slice_pass(c, j):
+            out_pass(c, j, j, x_codes[c], x_scales[c], w0_out[:], w0s_raw[:, H:N], True, False)
+
         def slice_passes(c, pair):
             for j in (2 * pair, 2 * pair + 1):
-                out_pass(c, j, j, x_codes[c], x_scales[c], w0_out[:], w0s_raw[:, H:N], True, False)
+                slice_pass(c, j)
 
         def unit_pass(c, g, j):
             u, at = (j // 2, 2 * g + j % 2) if c == 0 and g < 2 else (g, j)
-            out_pass(c, j, at, h_codes[c, u], h_scales[c, u], w1[:, g, :], w1s[:, g, :], False, g == 2)
+            out_pass(c, j, at, h_codes[c, u], h_scales[c, u], w1[:, g, :], w1s[:, g, :], False, g == (1 if (c, j) == (last, 2) else 2))
 
         def unit_passes(c, g, pair):
             for j in (2 * pair, 2 * pair + 1):
@@ -424,27 +427,38 @@ def tile_spn_w4_kernel(tc, x_bytes, x_scale, w0_words, w0_scales, w1_words, w1_s
                 unit_passes(c, 2, 1)
 
         c = last
-        for pair in range(2):
-            slice_passes(c, pair)
+        slice_pass(c, 0)
+        slice_pass(c, 2)
+        slice_pass(c, 3)
         h_quantize(c, 0)
         pool_weave(c, 1, 0, POOL_TOKENS[c])
         weave(nc.scalar.copy, c, 1, POOL_TOKENS[c], PAIR)
         weave(nc.scalar.copy, c, 1, PAIR, CHUNK)
-        for j in (2, 3):
-            weave(nc.scalar.copy, c, 2, P * j, P * (j + 1))
+        weave(nc.scalar.copy, c, 2, 2 * P, 3 * P)
+        weave(nc.scalar.copy, c, 2, 3 * P, CHUNK)
         relu_join(c)
         store(c - 1, 2)
         weave(nc.vector.tensor_copy, c, 2, 0, PAIR)
-        for pair in range(2):
-            unit_passes(c, 0, pair)
-        for g in (3, 1, 2):
-            h_quantize(c, g, 0, PAIR)
-            unit_passes(c, g, 0)
-        for g in (3, 1):
-            h_quantize(c, g, PAIR, CHUNK)
-            unit_passes(c, g, 1)
-        for j in (2, 3):
-            h_quantize(c, 2, P * j, P * (j + 1))
-            unit_pass(c, 2, j)
-        for j in (0, 2, 3):
-            store(c, j)
+        unit_pass(c, 0, 0)
+        unit_pass(c, 0, 2)
+        unit_pass(c, 0, 3)
+        slice_pass(c, 1)
+        unit_pass(c, 0, 1)
+        h_quantize(c, 3, 0 * P, 2 * P)
+        unit_passes(c, 3, 0)
+        h_quantize(c, 1, 0 * P, 2 * P)
+        unit_passes(c, 1, 0)
+        h_quantize(c, 2, 0 * P, 2 * P)
+        unit_passes(c, 2, 0)
+        h_quantize(c, 3, 2 * P, 4 * P)
+        unit_passes(c, 3, 1)
+        h_quantize(c, 2, 2 * P, 3 * P)
+        unit_pass(c, 2, 2)
+        h_quantize(c, 1, 2 * P, 4 * P)
+        unit_passes(c, 1, 1)
+        h_quantize(c, 2, 3 * P, 4 * P)
+        unit_pass(c, 2, 3)
+        store(c, 0)
+        store(c, 1)
+        store(c, 2)
+        store(c, 3)

@@ -32,8 +32,9 @@ N_CHUNKS = B // CHUNK
 PAIR = 2 * P
 PLANE_BANKS = 4
 PLANE_PAD = 16
-POOL_TOKENS = (192, 512, 512, 96)
-SCALAR_TOKENS = (96, 512, 512)
+POOL_HEAD = 2 * PASS * 3 // 16
+POOL_TAIL = PASS * 3 // 16
+SCALAR_HEAD = 96
 
 
 def tile_spn_w4_kernel(tc, x_bytes, x_scale, w0_words, w0_scales, w1_words, w1_scales, biases, out):
@@ -74,10 +75,6 @@ def tile_spn_w4_kernel(tc, x_bytes, x_scale, w0_words, w0_scales, w1_words, w1_s
         def load_w0(dst, n0, n1):
             nc.sync.dma_start(out=dst, in_=w0_words[0, :, 2 * n0 : 2 * n1])
 
-        def load_w0_scales(n0, n1):
-            for r in range(4):
-                nc.sync.dma_start(out=w0s_raw[r:P:32, n0:n1].bitcast(I32), in_=w0_scales[0, r:16:4, n0:n1].bitcast(I32))
-
         load_x(0, 1)
         load_x(1, 1)
         nc.sync.dma_start(out=xs_col[:], in_=x_scale.rearrange("o (p t) -> p (o t)", t=T))
@@ -85,7 +82,8 @@ def tile_spn_w4_kernel(tc, x_bytes, x_scale, w0_words, w0_scales, w1_words, w1_s
         load_w0(w0_lo[:, : 2 * PASS], 0, PASS)
         load_x(4, 2)
         load_w0(w0_lo[:, 2 * PASS :], PASS, 2 * PASS)
-        load_w0_scales(0, N)
+        for r in range(4):
+            nc.sync.dma_start(out=w0s_raw[r:P:32, :].bitcast(I32), in_=w0_scales[0, r:16:4, :].bitcast(I32))
         load_x(6, 4)
         nc.sync.dma_start(out=bias_h[:], in_=biases[0:H].rearrange("(g p t) -> p g t", g=G, p=P, t=T))
         load_w0(w0_hi[:], 2 * PASS, H)
@@ -97,7 +95,7 @@ def tile_spn_w4_kernel(tc, x_bytes, x_scale, w0_words, w0_scales, w1_words, w1_s
         nc.sync.dma_start(out=bias_o[:], in_=biases[H:N].partition_broadcast(P))
 
         x_wide, x_turned, x_woven, x_codes, x_scales = {}, {}, {}, {}, {}
-        h_planes, h_woven, h_codes, h_scales, sums, z_banks, z_pairs = {}, {}, {}, {}, {}, {}, {}
+        h_planes, h_woven, h_codes, h_scales, sums, z_banks, z_woven = {}, {}, {}, {}, {}, {}, {}
 
         def permute_words(raw, g0, g1, copy):
             copy(
@@ -135,7 +133,7 @@ def tile_spn_w4_kernel(tc, x_bytes, x_scale, w0_words, w0_scales, w1_words, w1_s
                     nc.tensor.transpose(bank[:, a, jj, :], words[:, a : X // 2 : 2], ident[:])
 
         def x_scale_out(c, j0, count):
-            if j0 == 0:
+            if c not in x_woven:
                 x_woven[c] = keep.tile([P, T * CHUNK], BF16, name="xg", tag="mid%d" % (c - 1), align_bytes=64)
             values = x_turned[c, j0][:].rearrange("p a j r -> p (a j r)").bitcast(BF16)
             nc.vector.tensor_tensor(
@@ -191,10 +189,10 @@ def tile_spn_w4_kernel(tc, x_bytes, x_scale, w0_words, w0_scales, w1_words, w1_s
                 plane(c, G - 1, t, P * i, bank[:, t, :])
 
         def vector_bank_out(c, i):
-            if i == 0:
-                z_pairs[c] = keep.tile([P, CHUNK, T], BF16, name="zg", bufs=2, align_bytes=64)
+            if c not in z_woven:
+                z_woven[c] = keep.tile([P, CHUNK, T], BF16, name="zg", bufs=2, align_bytes=64)
             nc.vector.tensor_tensor(
-                out=z_pairs[c][:, P * i : P * (i + 1), :],
+                out=z_woven[c][:, P * i : P * (i + 1), :],
                 in0=z_banks[c, i][:].rearrange("p t n -> p n t"),
                 in1=bias_h[:, G - 1, :].unsqueeze(1).to_broadcast([P, P, T]),
                 op=ADD,
@@ -203,36 +201,42 @@ def tile_spn_w4_kernel(tc, x_bytes, x_scale, w0_words, w0_scales, w1_words, w1_s
         def woven_view(c, g):
             key = 1 if g == 2 else g
             if (c, key) not in h_woven:
-                tag = ("mid%d" if c < last else "gate%d") % c if key == 1 else "gate%d" % (c + 1 if key else c)
-                h_woven[c, key] = keep.tile([P, T * CHUNK * (2 if key == 1 else 1)], BF16, name="hg", tag=tag, align_bytes=64)
+                if key == 0:
+                    tag = "gate%d" % c
+                elif key == 3:
+                    tag = "gate%d" % (c + 1)
+                elif c < last:
+                    tag = "mid%d" % c
+                else:
+                    tag = "gate%d" % c
+                width = T * CHUNK * (2 if key == 1 else 1)
+                h_woven[c, key] = keep.tile([P, width], BF16, name="hg", tag=tag, align_bytes=64)
             return h_woven[c, key][:, T * CHUNK * (g - key) :]
 
-        def relu_join(c):
+        def vector_relu(c):
             nc.vector.tensor_scalar(
                 out=woven_view(c, G - 1),
-                in0=z_pairs[c][:].rearrange("p n t -> p (n t)"),
+                in0=z_woven[c][:].rearrange("p n t -> p (n t)"),
                 scalar1=0.0,
                 scalar2=None,
                 op0=MAX,
             )
 
         def weave(copy, c, g, lo, hi):
-            if hi > lo:
-                copy(
-                    out=woven_view(c, g)[:, T * lo : T * hi].rearrange("p (c i t) -> p c t i", t=T, i=4),
-                    in_=planes_view(c, g)[:, :, lo:hi].rearrange("p t (c i) -> p c t i", i=4),
-                )
+            copy(
+                out=woven_view(c, g)[:, T * lo : T * hi].rearrange("p (c i t) -> p c t i", t=T, i=4),
+                in_=planes_view(c, g)[:, :, lo:hi].rearrange("p t (c i) -> p c t i", i=4),
+            )
 
         def pool_weave(c, g, lo, hi):
-            if hi > lo:
-                nc.gpsimd.tensor_scalar(
-                    out=woven_view(c, g)[:, T * lo : T * hi].rearrange("p (n t) -> p n t", t=T),
-                    in0=planes_view(c, g)[:, :, lo:hi].rearrange("p t n -> p n t"),
-                    scalar1=1.0,
-                    scalar2=0.0,
-                    op0=MULT,
-                    op1=ADD,
-                )
+            nc.gpsimd.tensor_scalar(
+                out=woven_view(c, g)[:, T * lo : T * hi].rearrange("p (n t) -> p n t", t=T),
+                in0=planes_view(c, g)[:, :, lo:hi].rearrange("p t n -> p n t"),
+                scalar1=1.0,
+                scalar2=0.0,
+                op0=MULT,
+                op1=ADD,
+            )
 
         def h_quantize(c, g, lo=0, hi=CHUNK):
             if (c, g) not in h_codes:
@@ -275,7 +279,8 @@ def tile_spn_w4_kernel(tc, x_bytes, x_scale, w0_words, w0_scales, w1_words, w1_s
 
         def unit_pass(c, g, j):
             u, at = (j // 2, 2 * g + j % 2) if c == 0 and g < 2 else (g, j)
-            out_pass(c, j, at, h_codes[c, u], h_scales[c, u], w1[:, g, :], w1s[:, g, :], False, g == (1 if (c, j) == (last, 2) else 2))
+            closing = 1 if (c, j) == (last, 2) else 2
+            out_pass(c, j, at, h_codes[c, u], h_scales[c, u], w1[:, g, :], w1s[:, g, :], False, g == closing)
 
         def unit_passes(c, g, pair):
             for j in (2 * pair, 2 * pair + 1):
@@ -283,7 +288,7 @@ def tile_spn_w4_kernel(tc, x_bytes, x_scale, w0_words, w0_scales, w1_words, w1_s
 
         def store(c, j0):
             tag, count, place = sum_place(c, j0)
-            res = keep.tile([P, count, OS], F32, name="res", bufs=4)
+            res = keep.tile([P, count, OS], F32, name="res%d_%d" % (c, j0))
             nc.vector.tensor_tensor(out=res[:], in0=sums[c, tag][:], in1=bias_o[:].unsqueeze(1).to_broadcast([P, count, OS]), op=ADD)
             nc.sync.dma_start(out=out_view[:, TILES * c + j0 : TILES * c + j0 + count, :], in_=res[:])
 
@@ -323,28 +328,29 @@ def tile_spn_w4_kernel(tc, x_bytes, x_scale, w0_words, w0_scales, w1_words, w1_s
         for i in range(2):
             scalar_short_planes(0, 1, 2 * i, 2)
             vector_bank(0, i, tags[i])
-        vector_bank_out(0, 0)
         vector_bank_out(0, 1)
+        vector_bank_out(0, 0)
         x_quantize(1, 0, CHUNK)
         h_quantize(0, 0)
         for i in range(2):
             scalar_short_planes(1, 1, 2 * i, 2)
             vector_bank(0, 2 + i, tags[2 + i])
-        pool_weave(0, 1, 0, POOL_TOKENS[0])
-        for i in range(2, 4):
-            vector_bank_out(0, i)
+        pool_weave(0, 1, 0, POOL_HEAD)
+        vector_bank_out(0, 3)
+        vector_bank_out(0, 2)
         for t in range(T):
             scalar_plane(0, 2, t)
-        x_cast(3, 0, 2, nc.scalar.copy)
-        weave(nc.scalar.copy, 0, 1, 2 * CHUNK - SCALAR_TOKENS[0], 2 * CHUNK)
+        x_cast(last, 0, 2, nc.scalar.copy)
+        weave(nc.scalar.copy, 0, 2, CHUNK - SCALAR_HEAD, CHUNK)
 
         for c in range(last):
             d = c + 1
             banks = side_banks(d)
             if c == 0:
-                weave(nc.vector.tensor_copy, c, 1, POOL_TOKENS[c], CHUNK)
-            relu_join(c)
-            weave(nc.vector.tensor_copy, c, 1, max(POOL_TOKENS[c], CHUNK), 2 * CHUNK - SCALAR_TOKENS[c])
+                weave(nc.vector.tensor_copy, c, 1, POOL_HEAD, CHUNK)
+            vector_relu(c)
+            if c == 0:
+                weave(nc.vector.tensor_copy, c, 2, 0, CHUNK - SCALAR_HEAD)
             h_quantize(c, 1)
             h_quantize(c, 3)
             h_quantize(c, 2)
@@ -375,30 +381,29 @@ def tile_spn_w4_kernel(tc, x_bytes, x_scale, w0_words, w0_scales, w1_words, w1_s
                     unit_passes(c, g, 0)
                 scalar_plane(d, 2, 0)
                 unit_passes(c, 2, 0)
-                x_scale_out(d + 1, 0, 2)
+                x_scale_out(d + 1, 2, 2)
                 scalar_plane(d, 2, 1)
-                vector_bank(d, 0, banks[0])
+                vector_bank(d, 0, banks[1])
                 scalar_plane(d, 2, 2)
                 unit_passes(c, 1, 1)
                 scalar_plane(d, 2, 3)
-                x_scale_out(d + 1, 2, 2)
-                vector_bank(d, 1, banks[1])
+                x_scale_out(d + 1, 0, 2)
+                vector_bank(d, 1, banks[0])
                 unit_passes(c, 3, 1)
                 store(c, 0)
                 vector_bank(d, 2, banks[2])
                 unit_passes(c, 2, 1)
                 x_quantize(d + 1, 0, CHUNK)
                 h_quantize(d, 0)
-                pool_weave(d, 1, 0, POOL_TOKENS[d])
+                pool_weave(d, 1, 0, CHUNK)
                 if d == 1:
-                    x_cast(3, 2, 2, nc.scalar.copy)
-                weave(nc.scalar.copy, d, 1, POOL_TOKENS[d], CHUNK)
-                weave(nc.scalar.copy, d, 1, 2 * CHUNK - SCALAR_TOKENS[d], 2 * CHUNK)
-                vector_bank_out(d, 0)
+                    x_cast(last, 2, 2, nc.scalar.copy)
+                weave(nc.scalar.copy, d, 2, 0, CHUNK)
+                vector_bank_out(d, 1)
                 scalar_plane(d + 1, 0, 0)
                 scalar_plane(d + 1, 0, 1)
                 vector_bank(d, 3, banks[0])
-                for i in range(1, 4):
+                for i in (0, 2, 3):
                     vector_bank_out(d, i)
                 store(c, 2)
                 for pair in range(2):
@@ -411,54 +416,46 @@ def tile_spn_w4_kernel(tc, x_bytes, x_scale, w0_words, w0_scales, w1_words, w1_s
                 scalar_plane(d, 1, 3)
                 unit_passes(c, 3, 0)
                 unit_passes(c, 2, 0)
-                vector_bank_out(d, 0)
                 vector_bank_out(d, 1)
+                vector_bank_out(d, 0)
                 store(c, 0)
                 scalar_plane(d, 2, 0)
-                vector_bank(d, 2, banks[0])
+                vector_bank(d, 2, banks[1])
                 vector_bank_out(d, 2)
                 scalar_plane(d, 2, 1)
-                vector_bank(d, 3, banks[1])
+                vector_bank(d, 3, banks[0])
                 vector_bank_out(d, 3)
                 scalar_plane(d, 2, 2)
                 scalar_plane(d, 2, 3)
-                unit_passes(c, 1, 1)
-                unit_passes(c, 3, 1)
-                unit_passes(c, 2, 1)
+                for g in (1, 3, 2):
+                    unit_passes(c, g, 1)
 
         c = last
-        slice_pass(c, 0)
-        slice_pass(c, 2)
-        slice_pass(c, 3)
+        for j in (0, 2, 3):
+            slice_pass(c, j)
         h_quantize(c, 0)
-        pool_weave(c, 1, 0, POOL_TOKENS[c])
-        weave(nc.scalar.copy, c, 1, POOL_TOKENS[c], PAIR)
+        pool_weave(c, 1, 0, POOL_TAIL)
+        weave(nc.scalar.copy, c, 1, POOL_TAIL, PAIR)
         weave(nc.scalar.copy, c, 1, PAIR, CHUNK)
-        weave(nc.scalar.copy, c, 2, 2 * P, 3 * P)
-        weave(nc.scalar.copy, c, 2, 3 * P, CHUNK)
-        relu_join(c)
+        for j in (2, 3):
+            weave(nc.scalar.copy, c, 2, P * j, P * (j + 1))
+        vector_relu(c)
         store(c - 1, 2)
         weave(nc.vector.tensor_copy, c, 2, 0, PAIR)
-        unit_pass(c, 0, 0)
-        unit_pass(c, 0, 2)
-        unit_pass(c, 0, 3)
+        for j in (0, 2, 3):
+            unit_pass(c, 0, j)
         slice_pass(c, 1)
         unit_pass(c, 0, 1)
-        h_quantize(c, 3, 0 * P, 2 * P)
-        unit_passes(c, 3, 0)
-        h_quantize(c, 1, 0 * P, 2 * P)
-        unit_passes(c, 1, 0)
-        h_quantize(c, 2, 0 * P, 2 * P)
-        unit_passes(c, 2, 0)
-        h_quantize(c, 3, 2 * P, 4 * P)
+        for g in (3, 1, 2):
+            h_quantize(c, g, 0, PAIR)
+            unit_passes(c, g, 0)
+        h_quantize(c, 3, PAIR, CHUNK)
         unit_passes(c, 3, 1)
         h_quantize(c, 2, 2 * P, 3 * P)
         unit_pass(c, 2, 2)
-        h_quantize(c, 1, 2 * P, 4 * P)
+        h_quantize(c, 1, PAIR, CHUNK)
         unit_passes(c, 1, 1)
-        h_quantize(c, 2, 3 * P, 4 * P)
+        h_quantize(c, 2, 3 * P, CHUNK)
         unit_pass(c, 2, 3)
-        store(c, 0)
-        store(c, 1)
-        store(c, 2)
-        store(c, 3)
+        for j in range(TILES):
+            store(c, j)

@@ -31,10 +31,10 @@ CHUNK = TILES * P
 N_CHUNKS = B // CHUNK
 PAIR = 2 * P
 PLANE_BANKS = 4
+SIDE_BANKS = 4
 PLANE_PAD = 16
-POOL_HEAD = 2 * PASS * 3 // 16
-POOL_TAIL = PASS * 3 // 16
-SCALAR_HEAD = 96
+POOL_HEAD = 400
+POOL_TAIL = 96
 
 
 def tile_spn_w4_kernel(tc, x_bytes, x_scale, w0_words, w0_scales, w1_words, w1_scales, biases, out):
@@ -53,18 +53,27 @@ def tile_spn_w4_kernel(tc, x_bytes, x_scale, w0_words, w0_scales, w1_words, w1_s
         w0_hi = keep.tile([P, 4 * PASS], U8, name="w0_hi", tag="gate0", align_bytes=64)
         w0_out = keep.tile([P, 2 * OS], U8, name="w0_out", align_bytes=64)
         w0_perm = keep.tile([P, 2 * H], U8, name="w0_perm", align_bytes=64)
-        w0s_raw = keep.tile([P, N], U8, name="w0s_raw", align_bytes=64)
-        w0s_perm = keep.tile([P, H], U8, name="w0s_perm", align_bytes=64)
+        s_raw = keep.tile([P, 2 * PASS], U8, name="s_raw", align_bytes=64)
+        s_lo = keep.tile([P, 2 * PASS], U8, name="s_lo", align_bytes=64)
+        s_hi = keep.tile([P, 2 * PASS], U8, name="s_hi", align_bytes=64)
         w1 = keep.tile([P, G, 2 * OS], U8, name="w1", align_bytes=64)
-        w1s = keep.tile([P, G, OS], U8, name="w1s", align_bytes=64)
+        s_out = keep.tile([P, G + 1, OS], U8, name="s_out", align_bytes=64)
         bias_h = keep.tile([P, G, T], BF16, name="bias_h")
         bias_o = keep.tile([P, OS], BF16, name="bias_o")
         xs_col = keep.tile([P, T], F32, name="xs_col")
-        x_raw = {}
 
-        nc.vector.memset(w0s_raw[:].bitcast(I32), 0)
-        nc.vector.memset(w1s[:].rearrange("p g n -> p (g n)").bitcast(I32), 0)
+        nc.vector.memset(s_raw[:].bitcast(I32), 0)
+        nc.vector.memset(s_hi[:].bitcast(I32), 0)
+        nc.vector.memset(s_out[:].rearrange("p g n -> p (g n)").bitcast(I32), 0)
         make_identity(nc, ident[:])
+
+        lists = {"sync": [], "tensor": [], "scalar": [], "vector": [], "pool": []}
+
+        def step(engine, key, needs, call, *args):
+            lists[engine].append((key, list(needs), call, args))
+
+        x_raw, x_wide, x_woven, x_codes, x_scales = {}, {}, {}, {}, {}
+        h_planes, h_woven, h_codes, h_scales, z_pairs, banks = {}, {}, {}, {}, {}, {}
 
         def load_x(j0, count):
             raw = keep.tile([P, count, X], U8, name="xbytes%d" % j0, align_bytes=64)
@@ -72,30 +81,47 @@ def tile_spn_w4_kernel(tc, x_bytes, x_scale, w0_words, w0_scales, w1_words, w1_s
                 x_raw[j0 + jj] = (raw, jj)
             nc.sync.dma_start(out=raw[:], in_=x_view[:, j0 : j0 + count, :])
 
-        def load_w0(dst, n0, n1):
-            nc.sync.dma_start(out=dst, in_=w0_words[0, :, 2 * n0 : 2 * n1])
+        def load(dst, src):
+            nc.sync.dma_start(out=dst, in_=src)
 
-        load_x(0, 1)
-        load_x(1, 1)
-        nc.sync.dma_start(out=xs_col[:], in_=x_scale.rearrange("o (p t) -> p (o t)", t=T))
-        load_x(2, 2)
-        load_w0(w0_lo[:, : 2 * PASS], 0, PASS)
-        load_x(4, 2)
-        load_w0(w0_lo[:, 2 * PASS :], PASS, 2 * PASS)
-        for r in range(4):
-            nc.sync.dma_start(out=w0s_raw[r:P:32, :].bitcast(I32), in_=w0_scales[0, r:16:4, :].bitcast(I32))
-        load_x(6, 4)
-        nc.sync.dma_start(out=bias_h[:], in_=biases[0:H].rearrange("(g p t) -> p g t", g=G, p=P, t=T))
-        load_w0(w0_hi[:], 2 * PASS, H)
-        load_x(10, 6)
-        load_w0(w0_out[:], H, N)
-        nc.sync.dma_start(out=w1[:], in_=w1_words.rearrange("g p n -> p g n"))
-        for r in range(4):
-            nc.sync.dma_start(out=w1s[r:P:32].bitcast(I32), in_=w1_scales[:, r:16:4, :].rearrange("g q n -> q g n").bitcast(I32))
-        nc.sync.dma_start(out=bias_o[:], in_=biases[H:N].partition_broadcast(P))
+        def w0_cols(n0, n1):
+            return w0_words[0, :, 2 * n0 : 2 * n1]
 
-        x_wide, x_turned, x_woven, x_codes, x_scales = {}, {}, {}, {}, {}
-        h_planes, h_woven, h_codes, h_scales, sums, z_banks, z_woven = {}, {}, {}, {}, {}, {}, {}
+        def load_hidden_scales():
+            for q in range(4):
+                rows = w0_scales[0, 4 * q : 4 * q + 4, 0:H].bitcast(I32).rearrange("r (h n) -> h r n", h=2)
+                nc.sync.dma_start(out=s_raw[32 * q : 32 * q + 8, :].bitcast(I32), in_=rows)
+
+        def move_hi_scales():
+            for r in range(4):
+                nc.sync.dma_start(out=s_hi[r:P:32, :].bitcast(I32), in_=s_lo[4 + r : P : 32, :].bitcast(I32))
+
+        def load_out_scales():
+            for r in range(4):
+                nc.sync.dma_start(out=s_out[r:P:32, G, :].bitcast(I32), in_=w0_scales[0, r:16:4, H:N].bitcast(I32))
+            for r in range(4):
+                nc.sync.dma_start(out=s_out[r:P:32, 0:G, :].bitcast(I32), in_=w1_scales[:, r:16:4, :].rearrange("g q n -> q g n").bitcast(I32))
+
+        x_loads = ((0, 1), (1, 1), (2, 2), (4, 2), (6, 2), (8, 2), (10, 6))
+        x_load_of = {j0 + jj: ("x", j0) for j0, count in x_loads for jj in range(count)}
+        step("sync", ("x", 0), [], load_x, 0, 1)
+        step("sync", ("x", 1), [], load_x, 1, 1)
+        step("sync", ("x", 2), [], load_x, 2, 2)
+        step("sync", ("w0", 0), [], load, w0_lo[:, : 2 * PASS], w0_cols(0, PASS))
+        step("sync", "xs", [], load, xs_col[:], x_scale.rearrange("o (p t) -> p (o t)", t=T))
+        step("sync", ("x", 4), [], load_x, 4, 2)
+        step("sync", ("x", 6), [], load_x, 6, 2)
+        step("sync", "s_raw", [], load_hidden_scales)
+        step("sync", ("w0", 1), [], load, w0_lo[:, 2 * PASS :], w0_cols(PASS, 2 * PASS))
+        step("sync", "bias_h", [], load, bias_h[:], biases[0:H].rearrange("(g p t) -> p g t", g=G, p=P, t=T))
+        step("sync", ("x", 8), [], load_x, 8, 2)
+        step("sync", ("w0", 2), [], load, w0_hi[:], w0_cols(2 * PASS, H))
+        step("sync", "s_hi", [("scales", 1)], move_hi_scales)
+        step("sync", ("x", 10), [], load_x, 10, 6)
+        step("sync", "w0_out", [], load, w0_out[:], w0_cols(H, N))
+        step("sync", "w1", [], load, w1[:], w1_words.rearrange("g p n -> p g n"))
+        step("sync", "s_out", [], load_out_scales)
+        step("sync", "bias_o", [], load, bias_o[:], biases[H:N].partition_broadcast(P))
 
         def permute_words(raw, g0, g1, copy):
             copy(
@@ -103,41 +129,59 @@ def tile_spn_w4_kernel(tc, x_bytes, x_scale, w0_words, w0_scales, w1_words, w1_s
                 in_=raw.bitcast(U16).rearrange("p (g m t) -> p g t m", t=T, m=P),
             )
 
-        def permute_scales(g0, g1):
-            cols = slice(PASS * g0, PASS * g1)
+        def permute_scales(g):
+            cols = slice(PASS * g, PASS * (g + 1))
             nc.vector.tensor_copy(
-                out=w0s_perm[:, cols].rearrange("p (g t m) -> p g t m", t=T, m=P),
-                in_=w0s_raw[:, cols].rearrange("p (g m t) -> p g t m", t=T, m=P),
+                out=s_lo[:, cols].rearrange("p (t m) -> p t m", t=T),
+                in_=s_raw[:, cols].rearrange("p (m t) -> p t m", t=T),
             )
 
-        def x_cast(c, j0, count, cast):
-            wide = keep.tile([P, count, X], BF16, name="xv%d_%d" % (c, j0), align_bytes=64)
-            for jj in range(count):
-                x_wide[c, j0 + jj] = wide[:, jj, :]
-            raw, first = x_raw[TILES * c + j0]
-            cast(
-                out=wide[:].rearrange("p j k -> p (j k)"),
-                in_=raw[:, first : first + count, :].rearrange("p j k -> p (j k)").bitcast(FP8),
-            )
+        def wide_tile(j0, count):
+            wide = keep.tile([P, count, X], BF16, name="xv%d" % j0, align_bytes=64)
+            raw, first = x_raw[j0]
+            return wide, raw[:, first : first + count, :].bitcast(FP8)
 
-        def scalar_first_cast(out, in_):
-            nc.scalar.activation(out=out[:, :P], in_=in_[:, :P], func=COPY)
-            nc.scalar.copy(out=out[:, P:], in_=in_[:, P:])
-
-        def x_transpose(c, j0, count, tag):
-            bank = psum.tile([P, 2, count, P], F32, name="xt", tag=tag, bufs=1)
-            x_turned[c, j0] = bank
+        def halves_apart(j0, count, wide):
             for jj in range(count):
-                words = x_wide[c, j0 + jj].bitcast(F32)
+                words = wide[:, jj, :].bitcast(F32)
+                x_wide[j0 + jj] = (words[:, :P], words[:, P:])
+
+        def scalar_cast(j0, count):
+            wide, codes = wide_tile(j0, count)
+            halves_apart(j0, count, wide)
+            nc.scalar.copy(out=wide[:].rearrange("p j (a m e) -> p j a m e", a=2, e=2), in_=codes.rearrange("p j (m a e) -> p j a m e", a=2, e=2))
+
+        def vector_cast(j):
+            wide, codes = wide_tile(j, 1)
+            halves_apart(j, 1, wide)
+            nc.vector.tensor_copy(out=wide[:, 0, :].rearrange("p (a m e) -> p m a e", a=2, e=2), in_=codes[:, 0, :].rearrange("p (m a e) -> p m a e", a=2, e=2))
+
+        def scalar_first_cast(j):
+            wide, codes = wide_tile(j, 1)
+            words = wide[:, 0, :].bitcast(F32)
+            x_wide[j] = (words[:, 0 : X // 2 : 2], words[:, 1 : X // 2 : 2])
+            nc.scalar.activation(out=wide[:, 0, :P], in_=codes[:, 0, :P], func=COPY)
+            nc.scalar.copy(out=wide[:, 0, P:], in_=codes[:, 0, P:])
+
+        side_tag = {}
+
+        def side_bank(job, shape, name):
+            banks[job] = psum.tile(shape, F32, name=name, tag=side_tag[job], bufs=1)
+            return banks[job]
+
+        def x_transpose(j0, count):
+            bank = side_bank(("xt", j0), [P, 2, count, P], "xt")
+            for jj in range(count):
                 for a in range(2):
-                    nc.tensor.transpose(bank[:, a, jj, :], words[:, a : X // 2 : 2], ident[:])
+                    nc.tensor.transpose(bank[:, a, jj, :], x_wide[j0 + jj][a], ident[:])
 
-        def x_scale_out(c, j0, count):
+        def x_scale_out(j0, count):
+            c, at = divmod(j0, TILES)
             if c not in x_woven:
                 x_woven[c] = keep.tile([P, T * CHUNK], BF16, name="xg", tag="mid%d" % (c - 1), align_bytes=64)
-            values = x_turned[c, j0][:].rearrange("p a j r -> p (a j r)").bitcast(BF16)
+            values = banks["xt", j0][:].rearrange("p a j r -> p (a j r)").bitcast(BF16)
             nc.vector.tensor_tensor(
-                out=x_woven[c][:, T * P * j0 : T * P * (j0 + count)].rearrange("p (r a e) -> p r a e", a=2, e=2),
+                out=x_woven[c][:, T * P * at : T * P * (at + count)].rearrange("p (r a e) -> p r a e", a=2, e=2),
                 in0=values.rearrange("p (a r e) -> p r a e", a=2, e=2),
                 in1=xs_col[:].rearrange("p (o a e) -> p o a e", o=1, a=2).to_broadcast([P, count * P, 2, 2]),
                 op=MULT,
@@ -151,311 +195,425 @@ def tile_spn_w4_kernel(tc, x_bytes, x_scale, w0_words, w0_scales, w1_words, w1_s
 
         def plane(c, g, t, lo, z):
             m0 = PASS * g + P * t
+            s0 = PASS * (g % 2) + P * t
             cols = slice(lo, lo + z.shape[1])
             nc.tensor.matmul_mx(
                 out=z,
                 lhsT=w0_perm[:, 2 * m0 : 2 * (m0 + P)].bitcast(FP4X4),
-                lhsT_scale=w0s_perm[:, m0 : m0 + P],
+                lhsT_scale=(s_lo, s_hi)[g // 2][:, s0 : s0 + P],
                 rhs=x_codes[c][:, cols].bitcast(FP8X4),
                 rhs_scale=x_scales[c][:, cols],
                 start=True,
                 stop=True,
             )
 
-        def planes_view(c, g):
-            first = min(g, 1)
-            if (c, first) not in h_planes:
-                width = CHUNK * (1 + first) + PLANE_PAD
-                h_planes[c, first] = keep.tile([P, T, width], BF16, name="hp%d_%d" % (c, first), align_bytes=64)
-            return h_planes[c, first][:, :, CHUNK * (g - first) :]
+        def planes_view(c, u):
+            if (c, u) not in h_planes:
+                h_planes[c, u] = keep.tile([P, T, CHUNK + PLANE_PAD], BF16, name="hp%d_%d" % (c, u), align_bytes=64)
+            return h_planes[c, u]
 
-        def scalar_plane(c, g, t):
-            bank = psum.tile([P, CHUNK], F32, name="z", bufs=PLANE_BANKS)
-            plane(c, g, t, 0, bank[:])
-            nc.scalar.activation(out=planes_view(c, g)[:, t, :CHUNK], in_=bank[:], func=RELU, bias=bias_h[:, g, t : t + 1])
-
-        def scalar_short_planes(g, pair, t0, count):
-            bank = psum.tile([P, count, PAIR], F32, name="z", bufs=PLANE_BANKS)
+        def ring_fill(job):
+            c, g, t0, count, lo, width = job
+            banks[job] = psum.tile([P, count, width], F32, name="z", bufs=PLANE_BANKS)
             for i in range(count):
-                plane(0, g, t0 + i, PAIR * pair, bank[:, i, :])
+                plane(c, g, t0 + i, lo, banks[job][:, i, :])
+
+        def ring_out(job):
+            c, g, t0, count, lo, width = job
+            u, at = (lo // PAIR, PAIR * g) if c == 0 and g < 2 else (g, 0)
             for i in range(count):
                 t = t0 + i
-                nc.scalar.activation(out=planes_view(0, pair)[:, t, PAIR * g : PAIR * (g + 1)], in_=bank[:, i, :], func=RELU, bias=bias_h[:, g, t : t + 1])
+                nc.scalar.activation(out=planes_view(c, u)[:, t, at : at + width], in_=banks[job][:, i, :], func=RELU, bias=bias_h[:, g, t : t + 1])
 
-        def vector_bank(c, i, tag):
-            bank = psum.tile([P, T, P], F32, name="zv", tag=tag, bufs=1)
-            z_banks[c, i] = bank
-            for t in range(T):
-                plane(c, G - 1, t, P * i, bank[:, t, :])
+        def pair_fill(c, g, i):
+            pair, a = divmod(i, 2)
+            bank = side_bank(("zv", c, g, i), [P, 2, PAIR], "zv")
+            for e in range(2):
+                plane(c, g, 2 * a + e, PAIR * pair, bank[:, e, :])
 
-        def vector_bank_out(c, i):
-            if c not in z_woven:
-                z_woven[c] = keep.tile([P, CHUNK, T], BF16, name="zg", bufs=2, align_bytes=64)
+        def pair_out(c, g, i):
+            pair, a = divmod(i, 2)
+            if (c, g) not in z_pairs:
+                z_pairs[c, g] = keep.tile([P, 2, 2 * CHUNK + PLANE_PAD], BF16, name="zg%d_%d" % (c, g), align_bytes=64)
             nc.vector.tensor_tensor(
-                out=z_woven[c][:, P * i : P * (i + 1), :],
-                in0=z_banks[c, i][:].rearrange("p t n -> p n t"),
-                in1=bias_h[:, G - 1, :].unsqueeze(1).to_broadcast([P, P, T]),
+                out=z_pairs[c, g][:, a, 2 * PAIR * pair : 2 * PAIR * (pair + 1)].rearrange("p (n e) -> p n e", e=2),
+                in0=banks["zv", c, g, i][:].rearrange("p e n -> p n e"),
+                in1=bias_h[:, g, 2 * a : 2 * a + 2].unsqueeze(1).to_broadcast([P, PAIR, 2]),
                 op=ADD,
             )
 
-        def woven_view(c, g):
-            key = 1 if g == 2 else g
-            if (c, key) not in h_woven:
-                if key == 0:
-                    tag = "gate%d" % c
-                elif key == 3:
-                    tag = "gate%d" % (c + 1)
-                elif c < last:
-                    tag = "mid%d" % c
-                else:
-                    tag = "gate%d" % c
-                width = T * CHUNK * (2 if key == 1 else 1)
-                h_woven[c, key] = keep.tile([P, width], BF16, name="hg", tag=tag, align_bytes=64)
-            return h_woven[c, key][:, T * CHUNK * (g - key) :]
+        def woven_tag(c, u):
+            if u == 0:
+                return "gate%d" % c
+            if u == G - 1:
+                return "gate%d" % (c + 1)
+            if u == 1:
+                return "mid%d" % c if c < last else "gate%d" % c
+            return "third%d" % c
 
-        def vector_relu(c):
+        def woven_view(c, u):
+            if (c, u) not in h_woven:
+                h_woven[c, u] = keep.tile([P, T * CHUNK], BF16, name="hg", tag=woven_tag(c, u), align_bytes=64)
+            return h_woven[c, u]
+
+        def vector_relu(c, g, lo):
             nc.vector.tensor_scalar(
-                out=woven_view(c, G - 1),
-                in0=z_woven[c][:].rearrange("p n t -> p (n t)"),
+                out=woven_view(c, g)[:, T * lo :].rearrange("p (n a e) -> p n a e", a=2, e=2),
+                in0=z_pairs[c, g][:, :, 2 * lo : 2 * CHUNK].rearrange("p a (n e) -> p n a e", e=2),
                 scalar1=0.0,
                 scalar2=None,
                 op0=MAX,
             )
 
-        def weave(copy, c, g, lo, hi):
+        def weave(copy, c, u, lo, hi):
             copy(
-                out=woven_view(c, g)[:, T * lo : T * hi].rearrange("p (c i t) -> p c t i", t=T, i=4),
-                in_=planes_view(c, g)[:, :, lo:hi].rearrange("p t (c i) -> p c t i", i=4),
+                out=woven_view(c, u)[:, T * lo : T * hi].rearrange("p (c i t) -> p c t i", t=T, i=4),
+                in_=planes_view(c, u)[:, :, lo:hi].rearrange("p t (c i) -> p c t i", i=4),
             )
 
-        def pool_weave(c, g, lo, hi):
+        def pool_weave(c, u, lo, hi):
             nc.gpsimd.tensor_scalar(
-                out=woven_view(c, g)[:, T * lo : T * hi].rearrange("p (n t) -> p n t", t=T),
-                in0=planes_view(c, g)[:, :, lo:hi].rearrange("p t n -> p n t"),
+                out=woven_view(c, u)[:, T * lo : T * hi].rearrange("p (n t) -> p n t", t=T),
+                in0=planes_view(c, u)[:, :, lo:hi].rearrange("p t n -> p n t"),
                 scalar1=1.0,
                 scalar2=0.0,
                 op0=MULT,
                 op1=ADD,
             )
 
-        def h_quantize(c, g, lo=0, hi=CHUNK):
-            if (c, g) not in h_codes:
-                h_codes[c, g] = keep.tile([P, CHUNK], U32, name="hq%d_%d" % (c, g), align_bytes=64)
-                h_scales[c, g] = keep.tile([P, CHUNK], U8, name="hqs%d_%d" % (c, g), align_bytes=64)
-            nc.vector.quantize_mx(out=h_codes[c, g][:, lo:hi].bitcast(FP8X4), scales=h_scales[c, g][:, lo:hi], in_=woven_view(c, g)[:, T * lo : T * hi])
+        def h_quantize(c, u, lo, hi):
+            if (c, u) not in h_codes:
+                h_codes[c, u] = keep.tile([P, CHUNK], U32, name="hq%d_%d" % (c, u), align_bytes=64)
+                h_scales[c, u] = keep.tile([P, CHUNK], U8, name="hqs%d_%d" % (c, u), align_bytes=64)
+            nc.vector.quantize_mx(out=h_codes[c, u][:, lo:hi].bitcast(FP8X4), scales=h_scales[c, u][:, lo:hi], in_=woven_view(c, u)[:, T * lo : T * hi])
 
-        def side_banks(c):
-            ring = ("x1", "o1", "o0")
-            k = 2 * (c - 1)
-            return ("x0", ring[k % 3], ring[(k + 1) % 3], ring[(k + 2) % 3])
+        def sum_job(c, j):
+            return (("o", c, j), 1, 0) if c == last else (("o", c, j - j % 2), 2, j % 2)
 
-        def sum_place(c, j):
-            banks = side_banks(c + 1)
-            if c == last:
-                return (banks[2], banks[1], banks[3], banks[0])[j], 1, 0
-            return banks[2 + j // 2], 2, j % 2
+        def unit_place(c, g, j):
+            return (j // 2, 2 * g + j % 2) if c == 0 and g < 2 else (g, j)
 
-        def out_pass(c, j, at, codes, scales, w, w_scales, opens, closes):
-            tag, count, place = sum_place(c, j)
-            if opens and place == 0:
-                sums[c, tag] = psum.tile([P, count, OS], F32, name="o", tag=tag, bufs=1)
+        def out_pass(c, j, g, closes):
+            job, count, place = sum_job(c, j)
+            opens = g == G and place == 0
+            if opens:
+                side_bank(job, [P, count, OS], "o")
+            if g == G:
+                at, codes, scales, w = j, x_codes[c], x_scales[c], w0_out[:]
+            else:
+                u, at = unit_place(c, g, j)
+                codes, scales, w = h_codes[c, u], h_scales[c, u], w1[:, g, :]
             cols = slice(at * P, (at + 1) * P)
             nc.tensor.matmul_mx(
-                out=sums[c, tag][:, place, :],
+                out=banks[job][:, place, :],
                 lhsT=codes[:, cols].bitcast(FP8X4),
                 lhsT_scale=scales[:, cols],
                 rhs=w.bitcast(FP4X4),
-                rhs_scale=w_scales,
-                start=opens and place == 0,
-                stop=closes and place == count - 1,
+                rhs_scale=s_out[:, g, :],
+                start=opens,
+                stop=closes,
             )
 
-        def slice_pass(c, j):
-            out_pass(c, j, j, x_codes[c], x_scales[c], w0_out[:], w0s_raw[:, H:N], True, False)
-
-        def slice_passes(c, pair):
-            for j in (2 * pair, 2 * pair + 1):
-                slice_pass(c, j)
-
-        def unit_pass(c, g, j):
-            u, at = (j // 2, 2 * g + j % 2) if c == 0 and g < 2 else (g, j)
-            closing = 1 if (c, j) == (last, 2) else 2
-            out_pass(c, j, at, h_codes[c, u], h_scales[c, u], w1[:, g, :], w1s[:, g, :], False, g == closing)
-
-        def unit_passes(c, g, pair):
-            for j in (2 * pair, 2 * pair + 1):
-                unit_pass(c, g, j)
-
         def store(c, j0):
-            tag, count, place = sum_place(c, j0)
+            job, count, place = sum_job(c, j0)
             res = keep.tile([P, count, OS], F32, name="res%d_%d" % (c, j0))
-            nc.vector.tensor_tensor(out=res[:], in0=sums[c, tag][:], in1=bias_o[:].unsqueeze(1).to_broadcast([P, count, OS]), op=ADD)
+            nc.vector.tensor_tensor(out=res[:], in0=banks[job][:], in1=bias_o[:].unsqueeze(1).to_broadcast([P, count, OS]), op=ADD)
             nc.sync.dma_start(out=out_view[:, TILES * c + j0 : TILES * c + j0 + count, :], in_=res[:])
 
-        x_cast(0, 0, 1, nc.vector.tensor_copy)
-        x_cast(0, 1, 1, scalar_first_cast)
-        x_transpose(0, 0, 1, "o0")
-        x_transpose(0, 1, 1, "o1")
-        x_cast(0, 2, 2, nc.scalar.copy)
-        x_cast(1, 0, 2, nc.scalar.copy)
-        permute_words(w0_lo[:, 2 * PASS :], 1, 2, nc.scalar.copy)
-        x_cast(1, 2, 2, nc.scalar.copy)
-        x_cast(2, 0, 2, nc.scalar.copy)
-        permute_words(w0_lo[:, : 2 * PASS], 0, 1, nc.vector.tensor_copy)
-        x_transpose(0, 2, 2, "x0")
-        x_transpose(1, 0, 2, "x1")
-        x_scale_out(0, 0, 1)
-        x_scale_out(0, 1, 1)
-        permute_scales(0, 1)
-        x_quantize(0, 0, PAIR)
-        permute_scales(1, 2)
-        x_scale_out(0, 2, 2)
-        permute_words(w0_hi[:], 2, G, nc.vector.tensor_copy)
-        x_quantize(0, PAIR, CHUNK)
-        permute_scales(2, G)
-        scalar_short_planes(0, 0, 0, 1)
-        scalar_short_planes(0, 0, 1, 1)
-        scalar_short_planes(0, 0, 2, 2)
-        pool_weave(0, 0, 0, PAIR)
-        for t in (0, 2):
-            scalar_short_planes(1, 0, t, 2)
-        pool_weave(0, 0, PAIR, CHUNK)
-        x_cast(2, 2, 2, nc.scalar.copy)
-        x_transpose(1, 2, 2, "o0")
-        x_scale_out(1, 0, 2)
-        x_scale_out(1, 2, 2)
-        tags = ("o1", "x0", "x1", "o0")
-        for i in range(2):
-            scalar_short_planes(0, 1, 2 * i, 2)
-            vector_bank(0, i, tags[i])
-        vector_bank_out(0, 1)
-        vector_bank_out(0, 0)
-        x_quantize(1, 0, CHUNK)
-        h_quantize(0, 0)
-        for i in range(2):
-            scalar_short_planes(1, 1, 2 * i, 2)
-            vector_bank(0, 2 + i, tags[2 + i])
-        pool_weave(0, 1, 0, POOL_HEAD)
-        vector_bank_out(0, 3)
-        vector_bank_out(0, 2)
-        for t in range(T):
-            scalar_plane(0, 2, t)
-        x_cast(last, 0, 2, nc.scalar.copy)
-        weave(nc.scalar.copy, 0, 2, CHUNK - SCALAR_HEAD, CHUNK)
+        ring = []
 
+        def s_cast(j0, count):
+            step("scalar", ("cast", j0), [x_load_of[j0]], scalar_cast, j0, count)
+
+        def s_planes(c, g, t0, count, lo, width):
+            job = (c, g, t0, count, lo, width)
+            ring.append(job)
+            step("scalar", ("out", job), [("fill", job), "bias_h"], ring_out, job)
+
+        def s_unit(c, g):
+            for t in range(T):
+                s_planes(c, g, t, 1, 0, CHUNK)
+
+        def planes_done(c, u, lo):
+            if c == 0 and u < 2:
+                return ("out", (0, lo // PAIR, 2, 2, PAIR * u, PAIR))
+            if c == 0:
+                return ("out", (0, u, 2, 2, 0, PAIR))
+            return ("out", (c, u, T - 1, 1, 0, CHUNK))
+
+        gates = {}
+
+        def weave_step(engine, c, u, lo, hi):
+            needs = [planes_done(c, u, lo), planes_done(c, u, hi - 1)] + gates.get((c, u), [])
+            if engine == "pool":
+                step(engine, ("weave", c, u, lo), needs, pool_weave, c, u, lo, hi)
+            else:
+                copy = nc.scalar.copy if engine == "scalar" else nc.vector.tensor_copy
+                step(engine, ("weave", c, u, lo), needs, weave, copy, c, u, lo, hi)
+
+        gates[0, 0] = [("words", 2)]
+        for c in range(N_CHUNKS):
+            if c > 0:
+                gates[c, 0] = [("q", c - 1, G - 1, 0)]
+            gates[c, 1] = [("xq", c + 1, 0)] if c < last else [("q", c, 0, 0)]
+
+        step("scalar", ("cast", 1), [("x", 1)], scalar_first_cast, 1)
+        s_cast(2, 2)
+        s_cast(4, 2)
+        s_cast(6, 2)
+        step("scalar", ("words", 1), [("w0", 1)], permute_words, w0_lo[:, 2 * PASS :], 1, 2, nc.scalar.copy)
+        s_cast(8, 2)
+        s_planes(0, 0, 0, 1, 0, PAIR)
+        s_planes(0, 0, 1, 1, 0, PAIR)
+        s_planes(0, 0, 2, 2, 0, PAIR)
+        for t0 in (0, 2):
+            s_planes(0, 1, t0, 2, 0, PAIR)
+        for g in range(2):
+            for t0 in (0, 2):
+                s_planes(0, g, t0, 2, PAIR, PAIR)
+        for t0 in (0, 2):
+            s_planes(0, 2, t0, 2, 0, PAIR)
+        s_cast(10, 2)
+        s_cast(12, 2)
+        weave_step("scalar", 0, 2, 0, PAIR)
+        for c in range(1, N_CHUNKS):
+            for g in range(G - 1):
+                s_unit(c, g)
+            if c == 1:
+                s_cast(14, 2)
+            if c < last:
+                weave_step("scalar", c, 2, 0, CHUNK)
+        weave_step("scalar", last, 1, POOL_TAIL, PAIR)
+        weave_step("scalar", last, 1, PAIR, CHUNK)
+        for j in (2, 3):
+            weave_step("scalar", last, 2, P * j, P * (j + 1))
+
+        weave_step("pool", 0, 0, 0, PAIR)
+        weave_step("pool", 0, 0, PAIR, CHUNK)
+        weave_step("pool", 0, 1, 0, POOL_HEAD)
+        for c in range(1, N_CHUNKS):
+            weave_step("pool", c, 0, 0, CHUNK)
+            weave_step("pool", c, 1, 0, CHUNK if c < last else POOL_TAIL)
+
+        reads = []
+
+        def v_read(job, needs, call, *args):
+            reads.append(job)
+            step("vector", ("out", job), [("fill", job)] + needs, call, *args)
+
+        def v_x(j0, count):
+            v_read(("xt", j0), ["xs"], x_scale_out, j0, count)
+
+        def v_pair(c, i, g=G - 1):
+            v_read(("zv", c, g, i), ["bias_h"], pair_out, c, g, i)
+
+        def v_store(c, j0):
+            v_read(("o", c, j0), ["bias_o"], store, c, j0)
+
+        def v_xq(c, lo, hi):
+            needs = [key for key, n, f, a in lists["vector"] if key[0] == "out" and key[1][0] == "xt"]
+            step("vector", ("xq", c, lo), needs, x_quantize, c, lo, hi)
+
+        def v_q(c, u, lo=0, hi=CHUNK):
+            needs = [key for engine in ("scalar", "pool") for key, n, f, a in lists[engine] if key[:3] == ("weave", c, u) and a[-2] < hi and a[-1] > lo]
+            step("vector", ("q", c, u, lo), needs, h_quantize, c, u, lo, hi)
+
+        def v_relu(c, g=G - 1, lo=0):
+            step("vector", ("relu", c, g), [], vector_relu, c, g, lo)
+
+        step("vector", ("cast", 0), [("x", 0)], vector_cast, 0)
+        step("vector", ("words", 0), [("w0", 0)], permute_words, w0_lo[:, : 2 * PASS], 0, 1, nc.vector.tensor_copy)
+        v_x(0, 1)
+        v_x(1, 1)
+        step("vector", ("scales", 0), ["s_raw"], permute_scales, 0)
+        v_xq(0, 0, PAIR)
+        step("vector", ("scales", 1), [], permute_scales, 1)
+        v_x(2, 2)
+        step("vector", ("words", 2), [("w0", 2)], permute_words, w0_hi[:], 2, G, nc.vector.tensor_copy)
+        v_xq(0, PAIR, CHUNK)
+        v_x(4, 2)
+        v_x(6, 2)
+        v_pair(0, 0)
+        v_pair(0, 1)
+        v_xq(1, 0, CHUNK)
+        v_q(0, 0)
+        v_pair(0, 2)
+        v_pair(0, 3)
+        v_pair(0, 2, 2)
+        v_pair(0, 3, 2)
+        v_relu(0)
+        weave_step("vector", 0, 1, POOL_HEAD, CHUNK)
+        v_relu(0, 2, PAIR)
         for c in range(last):
             d = c + 1
-            banks = side_banks(d)
-            if c == 0:
-                weave(nc.vector.tensor_copy, c, 1, POOL_HEAD, CHUNK)
-            vector_relu(c)
-            if c == 0:
-                weave(nc.vector.tensor_copy, c, 2, 0, CHUNK - SCALAR_HEAD)
-            h_quantize(c, 1)
-            h_quantize(c, 3)
-            h_quantize(c, 2)
-            if c == 0:
-                scalar_plane(d, 0, 0)
-                slice_passes(c, 0)
-                scalar_plane(d, 0, 1)
-                x_transpose(d + 1, 0, 2, banks[0])
-                scalar_plane(d, 0, 2)
-                x_transpose(d + 1, 2, 2, banks[1])
-                scalar_plane(d, 0, 3)
-                unit_passes(c, 0, 0)
-                scalar_plane(d, 1, 0)
-                slice_passes(c, 1)
-                scalar_plane(d, 1, 1)
-                unit_passes(c, 0, 1)
-            else:
-                for pair in range(2):
-                    if d < last:
-                        x_transpose(d + 1, 2 * pair, 2, banks[pair])
-                    else:
-                        vector_bank(d, pair, banks[pair])
-                    scalar_plane(d, 1, pair)
-            pool_weave(d, 0, 0, CHUNK)
+            if c > 0:
+                v_relu(c)
+            for u in (1, 3, 2):
+                v_q(c, u)
             if d < last:
-                for t, g in ((2, 1), (3, 3)):
-                    scalar_plane(d, 1, t)
-                    unit_passes(c, g, 0)
-                scalar_plane(d, 2, 0)
-                unit_passes(c, 2, 0)
-                x_scale_out(d + 1, 2, 2)
-                scalar_plane(d, 2, 1)
-                vector_bank(d, 0, banks[1])
-                scalar_plane(d, 2, 2)
-                unit_passes(c, 1, 1)
-                scalar_plane(d, 2, 3)
-                x_scale_out(d + 1, 0, 2)
-                vector_bank(d, 1, banks[0])
-                unit_passes(c, 3, 1)
-                store(c, 0)
-                vector_bank(d, 2, banks[2])
-                unit_passes(c, 2, 1)
-                x_quantize(d + 1, 0, CHUNK)
-                h_quantize(d, 0)
-                pool_weave(d, 1, 0, CHUNK)
-                if d == 1:
-                    x_cast(last, 2, 2, nc.scalar.copy)
-                weave(nc.scalar.copy, d, 2, 0, CHUNK)
-                vector_bank_out(d, 1)
-                scalar_plane(d + 1, 0, 0)
-                scalar_plane(d + 1, 0, 1)
-                vector_bank(d, 3, banks[0])
-                for i in (0, 2, 3):
-                    vector_bank_out(d, i)
-                store(c, 2)
-                for pair in range(2):
-                    scalar_plane(d + 1, 0, 2 + pair)
-                    slice_passes(d, pair)
-                    unit_passes(d, 0, pair)
-            else:
-                unit_passes(c, 1, 0)
-                scalar_plane(d, 1, 2)
-                scalar_plane(d, 1, 3)
-                unit_passes(c, 3, 0)
-                unit_passes(c, 2, 0)
-                vector_bank_out(d, 1)
-                vector_bank_out(d, 0)
-                store(c, 0)
-                scalar_plane(d, 2, 0)
-                vector_bank(d, 2, banks[1])
-                vector_bank_out(d, 2)
-                scalar_plane(d, 2, 1)
-                vector_bank(d, 3, banks[0])
-                vector_bank_out(d, 3)
-                scalar_plane(d, 2, 2)
-                scalar_plane(d, 2, 3)
-                for g in (1, 3, 2):
-                    unit_passes(c, g, 1)
+                v_x(TILES * (d + 1), 2)
+                v_x(TILES * (d + 1) + 2, 2)
+                v_store(c, 0)
+                v_xq(d + 1, 0, CHUNK)
+                v_q(d, 0)
+                for i in range(4):
+                    v_pair(d, i)
+                v_store(c, 2)
+        v_pair(last, 0)
+        v_pair(last, 1)
+        v_store(last - 1, 0)
+        v_pair(last, 2)
+        v_pair(last, 3)
+        v_q(last, 0)
+        v_relu(last)
+        v_store(last - 1, 2)
+        weave_step("vector", last, 2, 0, PAIR)
+        for u in (3, 1, 2):
+            v_q(last, u, 0, PAIR)
+        v_q(last, 3, PAIR, CHUNK)
+        v_q(last, 1, PAIR, CHUNK)
+        v_q(last, 2, 2 * P, 3 * P)
+        v_store(last, 0)
+        v_q(last, 2, 3 * P, CHUNK)
+        for j in range(1, TILES):
+            v_store(last, j)
 
-        c = last
-        for j in (0, 2, 3):
-            slice_pass(c, j)
-        h_quantize(c, 0)
-        pool_weave(c, 1, 0, POOL_TAIL)
-        weave(nc.scalar.copy, c, 1, POOL_TAIL, PAIR)
-        weave(nc.scalar.copy, c, 1, PAIR, CHUNK)
-        for j in (2, 3):
-            weave(nc.scalar.copy, c, 2, P * j, P * (j + 1))
-        vector_relu(c)
-        store(c - 1, 2)
-        weave(nc.vector.tensor_copy, c, 2, 0, PAIR)
-        for j in (0, 2, 3):
-            unit_pass(c, 0, j)
-        slice_pass(c, 1)
-        unit_pass(c, 0, 1)
-        for g in (3, 1, 2):
-            h_quantize(c, g, 0, PAIR)
-            unit_passes(c, g, 0)
-        h_quantize(c, 3, PAIR, CHUNK)
-        unit_passes(c, 3, 1)
-        h_quantize(c, 2, 2 * P, 3 * P)
-        unit_pass(c, 2, 2)
-        h_quantize(c, 1, PAIR, CHUNK)
-        unit_passes(c, 1, 1)
-        h_quantize(c, 2, 3 * P, CHUNK)
-        unit_pass(c, 2, 3)
-        for j in range(TILES):
-            store(c, j)
+        opened = []
+        filled = []
+
+        def freed(job):
+            n = len(opened)
+            opened.append(job)
+            if n < SIDE_BANKS:
+                side_tag[job] = "side%d" % n
+                return []
+            side_tag[job] = side_tag[reads[n - SIDE_BANKS]]
+            return [("out", reads[n - SIDE_BANKS])]
+
+        def codes_of(key, lo, hi):
+            return [k for k, n, f, a in lists["vector"] if k[: len(key)] == key and a[-2] < hi and a[-1] > lo]
+
+        def weights_of(g):
+            return [("words", min(g, 2)), ("scales", g) if g < 2 else "s_hi"]
+
+        def t_x(j0, count):
+            casts = [("cast", j) for j in (j0, j0 + count - 1) if j < 2 or j % 2 == 0]
+            step("tensor", ("fill", ("xt", j0)), casts + freed(("xt", j0)), x_transpose, j0, count)
+
+        def t_planes(count):
+            for i in range(count):
+                n = len(filled)
+                job = ring[n]
+                filled.append(job)
+                c, g, t0, planes, lo, width = job
+                needs = codes_of(("xq", c), lo, lo + width) + weights_of(g)
+                if n >= PLANE_BANKS:
+                    needs.append(("out", ring[n - PLANE_BANKS]))
+                step("tensor", ("fill", job), needs, ring_fill, job)
+
+        def t_pair(c, i, g=G - 1):
+            lo = PAIR * (i // 2)
+            needs = codes_of(("xq", c), lo, lo + PAIR) + weights_of(g) + freed(("zv", c, g, i))
+            step("tensor", ("fill", ("zv", c, g, i)), needs, pair_fill, c, g, i)
+
+        def t_pass(c, j, g, closing=False):
+            job, count, place = sum_job(c, j)
+            if g == G:
+                needs = ["w0_out", "s_out"] + (freed(job) if place == 0 else [])
+            else:
+                u, at = unit_place(c, g, j)
+                needs = ["w1"] + codes_of(("q", c, u), P * at, P * (at + 1))
+            closes = closing and place == count - 1
+            step("tensor", ("fill", job) if closes else ("pass", c, j, g), needs, out_pass, c, j, g, closes)
+
+        def t_passes(c, pair, g, closing=False):
+            for j in (2 * pair, 2 * pair + 1):
+                t_pass(c, j, g, closing)
+
+        t_x(0, 1)
+        t_x(1, 1)
+        t_x(2, 2)
+        t_x(4, 2)
+        t_planes(5)
+        t_x(6, 2)
+        t_planes(1)
+        t_pair(0, 0)
+        t_planes(1)
+        t_pair(0, 1)
+        t_planes(2)
+        t_pair(0, 2)
+        t_planes(1)
+        t_pair(0, 3)
+        t_planes(1)
+        t_pair(0, 2, 2)
+        t_pair(0, 3, 2)
+        for c in range(last):
+            d = c + 1
+            t_planes(2)
+            if c > 0:
+                t_pair(c, 3)
+            t_planes(2)
+            if d < last:
+                t_x(TILES * (d + 1), 2)
+                t_x(TILES * (d + 1) + 2, 2)
+                t_passes(c, 0, G)
+                t_passes(c, 0, 0)
+                t_pair(d, 0)
+                t_planes(2)
+                t_passes(c, 0, 1)
+                t_planes(1)
+                t_passes(c, 0, 3)
+                t_planes(1)
+                t_passes(c, 0, 2, True)
+                for g in (G, 0, 1):
+                    t_planes(1)
+                    t_passes(c, 1, g)
+                t_planes(1)
+                t_pair(d, 1)
+                t_pair(d, 2)
+                t_passes(c, 1, 3)
+                t_passes(c, 1, 2, True)
+        c = last - 1
+        t_pair(last, 0)
+        t_pair(last, 1)
+        t_passes(c, 0, G)
+        t_passes(c, 0, 0)
+        t_planes(1)
+        t_pair(last, 2)
+        t_planes(1)
+        t_passes(c, 0, 1)
+        t_planes(1)
+        t_passes(c, 0, 3)
+        t_planes(1)
+        t_passes(c, 0, 2, True)
+        t_pair(last, 3)
+        for g in (G, 0, 1):
+            t_planes(1)
+            t_passes(c, 1, g)
+        t_planes(1)
+        t_passes(c, 1, 3)
+        t_passes(c, 1, 2, True)
+        for j in range(3):
+            t_pass(last, j, G)
+        for j in range(3):
+            t_pass(last, j, 0)
+        t_pass(last, 3, G)
+        t_pass(last, 3, 0)
+        for g in (3, 1):
+            t_passes(last, 0, g)
+        t_passes(last, 0, 2, True)
+        t_passes(last, 1, 3)
+        t_passes(last, 1, 1)
+        t_passes(last, 1, 2, True)
+
+        done = set()
+        at = {engine: 0 for engine in lists}
+        for sweep in range(sum(len(steps) for steps in lists.values())):
+            for engine, steps in lists.items():
+                for key, needs, call, args in steps[at[engine] :]:
+                    if not all(need in done for need in needs):
+                        break
+                    call(*args)
+                    done.add(key)
+                    at[engine] = at[engine] + 1
+        assert all(at[engine] == len(steps) for engine, steps in lists.items())

@@ -273,8 +273,8 @@ def tile_spn_w4_kernel(tc, x_bytes, x_scale, w0_words, w0_scales, w1_words, w1_s
 
         def pool_weave(c, u, lo, hi):
             nc.gpsimd.tensor_scalar(
-                out=woven_view(c, u)[:, T * lo : T * hi].rearrange("p (n t) -> p n t", t=T),
-                in0=planes_view(c, u)[:, :, lo:hi].rearrange("p t n -> p n t"),
+                out=woven_view(c, u)[:, T * lo : T * hi].rearrange("p (c i t) -> p c t i", t=T, i=4),
+                in0=planes_view(c, u)[:, :, lo:hi].rearrange("p t (c i) -> p c t i", i=4),
                 scalar1=1.0,
                 scalar2=0.0,
                 op0=MULT,
@@ -559,16 +559,15 @@ def tile_spn_w4_kernel(tc, x_bytes, x_scale, w0_words, w0_scales, w1_words, w1_s
                 t_passes(c, 0, G)
                 t_passes(c, 0, 0)
                 t_pair(d, 0)
-                t_planes(2)
+                t_planes(T)
                 t_passes(c, 0, 1)
-                t_planes(1)
                 t_passes(c, 0, 3)
-                t_planes(1)
                 t_passes(c, 0, 2, True)
-                for g in (G, 0, 1):
-                    t_planes(1)
-                    t_passes(c, 1, g)
+                t_planes(3)
+                t_passes(c, 1, G)
+                t_passes(c, 1, 0)
                 t_planes(1)
+                t_passes(c, 1, 1)
                 t_pair(d, 1)
                 t_pair(d, 2)
                 t_passes(c, 1, 3)
@@ -578,19 +577,21 @@ def tile_spn_w4_kernel(tc, x_bytes, x_scale, w0_words, w0_scales, w1_words, w1_s
         t_pair(last, 1)
         t_passes(c, 0, G)
         t_passes(c, 0, 0)
-        t_planes(1)
         t_pair(last, 2)
-        t_planes(1)
+        t_planes(2)
         t_passes(c, 0, 1)
         t_planes(1)
         t_passes(c, 0, 3)
         t_planes(1)
         t_passes(c, 0, 2, True)
-        t_pair(last, 3)
-        for g in (G, 0, 1):
-            t_planes(1)
-            t_passes(c, 1, g)
         t_planes(1)
+        t_pair(last, 3)
+        t_planes(1)
+        t_passes(c, 1, G)
+        t_planes(1)
+        t_passes(c, 1, 0)
+        t_planes(1)
+        t_passes(c, 1, 1)
         t_passes(c, 1, 3)
         t_passes(c, 1, 2, True)
         for j in range(3):

@@ -33,8 +33,9 @@ PAIR = 2 * P
 PLANE_BANKS = 4
 SIDE_BANKS = 4
 PLANE_PAD = 16
-POOL_HEAD = 400
-POOL_TAIL = 96
+POOL_HEAD = 448
+POOL_TAIL = 64
+VECTOR_HEAD = 64
 
 
 def tile_spn_w4_kernel(tc, x_bytes, x_scale, w0_words, w0_scales, w1_words, w1_scales, biases, out):
@@ -220,7 +221,7 @@ def tile_spn_w4_kernel(tc, x_bytes, x_scale, w0_words, w0_scales, w1_words, w1_s
 
         def ring_out(job):
             c, g, t0, count, lo, width = job
-            u, at = (lo // PAIR, PAIR * g) if c == 0 and g < 2 else (g, 0)
+            u, at = (lo // PAIR, PAIR * g) if c == 0 and g < 2 else (g, lo)
             for i in range(count):
                 t = t0 + i
                 nc.scalar.activation(out=planes_view(c, u)[:, t, at : at + width], in_=banks[job][:, i, :], func=RELU, bias=bias_h[:, g, t : t + 1])
@@ -330,8 +331,8 @@ def tile_spn_w4_kernel(tc, x_bytes, x_scale, w0_words, w0_scales, w1_words, w1_s
             ring.append(job)
             step("scalar", ("out", job), [("fill", job), "bias_h"], ring_out, job)
 
-        def s_unit(c, g):
-            for t in range(T):
+        def s_unit(c, g, planes=T):
+            for t in range(planes):
                 s_planes(c, g, t, 1, 0, CHUNK)
 
         def planes_done(c, u, lo):
@@ -339,6 +340,8 @@ def tile_spn_w4_kernel(tc, x_bytes, x_scale, w0_words, w0_scales, w1_words, w1_s
                 return ("out", (0, lo // PAIR, 2, 2, PAIR * u, PAIR))
             if c == 0:
                 return ("out", (0, u, 2, 2, 0, PAIR))
+            if (c, u) == (last - 1, 2):
+                return ("out", (c, u, T - 1, 1, lo - lo % PAIR, PAIR))
             return ("out", (c, u, T - 1, 1, 0, CHUNK))
 
         gates = {}
@@ -375,13 +378,20 @@ def tile_spn_w4_kernel(tc, x_bytes, x_scale, w0_words, w0_scales, w1_words, w1_s
             s_planes(0, 2, t0, 2, 0, PAIR)
         s_cast(10, 2)
         s_cast(12, 2)
-        weave_step("scalar", 0, 2, 0, PAIR)
+        weave_step("scalar", 0, 2, VECTOR_HEAD, PAIR)
         for c in range(1, N_CHUNKS):
-            for g in range(G - 1):
-                s_unit(c, g)
+            s_unit(c, 0)
+            s_unit(c, 1)
+            if c == last - 1:
+                s_unit(c, 2, T - 1)
+                for lo in (0, PAIR):
+                    s_planes(c, 2, T - 1, 1, lo, PAIR)
+                for lo in (0, PAIR):
+                    weave_step("scalar", c, 2, lo, lo + PAIR)
+            else:
+                s_unit(c, 2)
             if c == 1:
                 s_cast(14, 2)
-            if c < last:
                 weave_step("scalar", c, 2, 0, CHUNK)
         weave_step("scalar", last, 1, POOL_TAIL, PAIR)
         weave_step("scalar", last, 1, PAIR, CHUNK)
@@ -444,6 +454,7 @@ def tile_spn_w4_kernel(tc, x_bytes, x_scale, w0_words, w0_scales, w1_words, w1_s
         v_relu(0)
         weave_step("vector", 0, 1, POOL_HEAD, CHUNK)
         v_relu(0, 2, PAIR)
+        weave_step("vector", 0, 2, 0, VECTOR_HEAD)
         for c in range(last):
             d = c + 1
             if c > 0:
@@ -566,7 +577,7 @@ def tile_spn_w4_kernel(tc, x_bytes, x_scale, w0_words, w0_scales, w1_words, w1_s
                 t_planes(3)
                 t_passes(c, 1, G)
                 t_passes(c, 1, 0)
-                t_planes(1)
+                t_planes(d)
                 t_passes(c, 1, 1)
                 t_pair(d, 1)
                 t_pair(d, 2)

@@ -111,8 +111,8 @@ def tile_spn_w4_kernel(tc, x_bytes, x_scale, w0_words, w0_scales, w1_words, w1_s
         step("sync", ("w0", 0), [], load, w0_lo[:, : 2 * PASS], w0_cols(0, PASS))
         step("sync", "xs", [], load, xs_col[:], x_scale.rearrange("o (p t) -> p (o t)", t=T))
         step("sync", ("x", 4), [], load_x, 4, 2)
-        step("sync", ("x", 6), [], load_x, 6, 2)
         step("sync", "s_raw", [], load_hidden_scales)
+        step("sync", ("x", 6), [], load_x, 6, 2)
         step("sync", ("w0", 1), [], load, w0_lo[:, 2 * PASS :], w0_cols(PASS, 2 * PASS))
         step("sync", "bias_h", [], load, bias_h[:], biases[0:H].rearrange("(g p t) -> p g t", g=G, p=P, t=T))
         step("sync", ("x", 8), [], load_x, 8, 2)
@@ -159,10 +159,12 @@ def tile_spn_w4_kernel(tc, x_bytes, x_scale, w0_words, w0_scales, w1_words, w1_s
 
         def scalar_first_cast(j):
             wide, codes = wide_tile(j, 1)
-            words = wide[:, 0, :].bitcast(F32)
-            x_wide[j] = (words[:, 0 : X // 2 : 2], words[:, 1 : X // 2 : 2])
-            nc.scalar.activation(out=wide[:, 0, :P], in_=codes[:, 0, :P], func=COPY)
-            nc.scalar.copy(out=wide[:, 0, P:], in_=codes[:, 0, P:])
+            halves_apart(j, 1, wide)
+            halves = wide[:, 0, :].rearrange("p (a m e) -> p a m e", a=2, e=2)
+            pairs = codes[:, 0, :].rearrange("p (m a e) -> p a m e", a=2, e=2)
+            nc.scalar.activation(out=halves[:, 0, 0, :], in_=pairs[:, 0, 0, :], func=COPY)
+            nc.scalar.copy(out=halves[:, 0, 1:, :], in_=pairs[:, 0, 1:, :])
+            nc.scalar.copy(out=halves[:, 1], in_=pairs[:, 1])
 
         side_tag = {}
 
@@ -360,7 +362,7 @@ def tile_spn_w4_kernel(tc, x_bytes, x_scale, w0_words, w0_scales, w1_words, w1_s
                 gates[c, 0] = [("q", c - 1, G - 1, 0)]
             gates[c, 1] = [("xq", c + 1, 0)] if c < last else [("q", c, 0, 0)]
 
-        step("scalar", ("cast", 1), [("x", 1)], scalar_first_cast, 1)
+        step("scalar", ("cast", 0), [("x", 0)], scalar_first_cast, 0)
         s_cast(2, 2)
         s_cast(4, 2)
         s_cast(6, 2)
@@ -431,7 +433,7 @@ def tile_spn_w4_kernel(tc, x_bytes, x_scale, w0_words, w0_scales, w1_words, w1_s
         def v_relu(c, g=G - 1, lo=0):
             step("vector", ("relu", c, g), [], vector_relu, c, g, lo)
 
-        step("vector", ("cast", 0), [("x", 0)], vector_cast, 0)
+        step("vector", ("cast", 1), [("x", 1)], vector_cast, 1)
         step("vector", ("words", 0), [("w0", 0)], permute_words, w0_lo[:, : 2 * PASS], 0, 1, nc.vector.tensor_copy)
         v_x(0, 1)
         v_x(1, 1)

@@ -54,9 +54,9 @@ def tile_spn_w4_kernel(tc, x_bytes, x_scale, w0_words, w0_scales, w1_words, w1_s
         w0_hi = keep.tile([P, 4 * PASS], U8, name="w0_hi", tag="gate0", align_bytes=64)
         w0_out = keep.tile([P, 2 * OS], U8, name="w0_out", align_bytes=64)
         w0_perm = keep.tile([P, 2 * H], U8, name="w0_perm", align_bytes=64)
-        s_raw = keep.tile([P, 2 * PASS], U8, name="s_raw", align_bytes=64)
-        s_lo = keep.tile([P, 2 * PASS], U8, name="s_lo", align_bytes=64)
-        s_hi = keep.tile([P, 2 * PASS], U8, name="s_hi", align_bytes=64)
+        s_raw = keep.tile([P, PASS], U8, name="s_raw", align_bytes=64)
+        s_packed = keep.tile([P, PASS], U8, name="s_packed", align_bytes=64)
+        s_perm = keep.tile([P, G, PASS], U8, name="s_perm", align_bytes=64)
         w1 = keep.tile([P, G, 2 * OS], U8, name="w1", align_bytes=64)
         s_out = keep.tile([P, G + 1, OS], U8, name="s_out", align_bytes=64)
         bias_h = keep.tile([P, G, T], BF16, name="bias_h")
@@ -64,7 +64,7 @@ def tile_spn_w4_kernel(tc, x_bytes, x_scale, w0_words, w0_scales, w1_words, w1_s
         xs_col = keep.tile([P, T], F32, name="xs_col")
 
         nc.vector.memset(s_raw[:].bitcast(I32), 0)
-        nc.vector.memset(s_hi[:].bitcast(I32), 0)
+        nc.vector.memset(s_perm[:].rearrange("p g n -> p (g n)").bitcast(I32), 0)
         nc.vector.memset(s_out[:].rearrange("p g n -> p (g n)").bitcast(I32), 0)
         make_identity(nc, ident[:])
 
@@ -89,13 +89,12 @@ def tile_spn_w4_kernel(tc, x_bytes, x_scale, w0_words, w0_scales, w1_words, w1_s
             return w0_words[0, :, 2 * n0 : 2 * n1]
 
         def load_hidden_scales():
-            for q in range(4):
-                rows = w0_scales[0, 4 * q : 4 * q + 4, 0:H].bitcast(I32).rearrange("r (h n) -> h r n", h=2)
-                nc.sync.dma_start(out=s_raw[32 * q : 32 * q + 8, :].bitcast(I32), in_=rows)
+            rows = w0_scales[0, :, 0:H].bitcast(I32).rearrange("r (g n) -> r g n", g=G)
+            nc.sync.dma_start(out=s_raw[0 : 16 * G, :].bitcast(I32), in_=rows)
 
-        def move_hi_scales():
-            for r in range(4):
-                nc.sync.dma_start(out=s_hi[r:P:32, :].bitcast(I32), in_=s_lo[4 + r : P : 32, :].bitcast(I32))
+        def spread_scales():
+            for q in range(4):
+                nc.sync.dma_start(out=s_perm[32 * q : 32 * q + 4].bitcast(I32), in_=s_packed[16 * q : 16 * q + 16, :].bitcast(I32))
 
         def load_out_scales():
             for r in range(4):
@@ -107,17 +106,17 @@ def tile_spn_w4_kernel(tc, x_bytes, x_scale, w0_words, w0_scales, w1_words, w1_s
         x_load_of = {j0 + jj: ("x", j0) for j0, count in x_loads for jj in range(count)}
         step("sync", ("x", 0), [], load_x, 0, 1)
         step("sync", ("x", 1), [], load_x, 1, 1)
+        step("sync", "s_raw", [], load_hidden_scales)
         step("sync", ("x", 2), [], load_x, 2, 2)
         step("sync", ("w0", 0), [], load, w0_lo[:, : 2 * PASS], w0_cols(0, PASS))
         step("sync", "xs", [], load, xs_col[:], x_scale.rearrange("o (p t) -> p (o t)", t=T))
         step("sync", ("x", 4), [], load_x, 4, 2)
-        step("sync", "s_raw", [], load_hidden_scales)
         step("sync", ("x", 6), [], load_x, 6, 2)
         step("sync", ("w0", 1), [], load, w0_lo[:, 2 * PASS :], w0_cols(PASS, 2 * PASS))
         step("sync", "bias_h", [], load, bias_h[:], biases[0:H].rearrange("(g p t) -> p g t", g=G, p=P, t=T))
+        step("sync", "s_perm", ["scales"], spread_scales)
         step("sync", ("x", 8), [], load_x, 8, 2)
         step("sync", ("w0", 2), [], load, w0_hi[:], w0_cols(2 * PASS, H))
-        step("sync", "s_hi", [("scales", 1)], move_hi_scales)
         step("sync", ("x", 10), [], load_x, 10, 6)
         step("sync", "w0_out", [], load, w0_out[:], w0_cols(H, N))
         step("sync", "w1", [], load, w1[:], w1_words.rearrange("g p n -> p g n"))
@@ -130,12 +129,8 @@ def tile_spn_w4_kernel(tc, x_bytes, x_scale, w0_words, w0_scales, w1_words, w1_s
                 in_=raw.bitcast(U16).rearrange("p (g m t) -> p g t m", t=T, m=P),
             )
 
-        def permute_scales(g):
-            cols = slice(PASS * g, PASS * (g + 1))
-            nc.vector.tensor_copy(
-                out=s_lo[:, cols].rearrange("p (t m) -> p t m", t=T),
-                in_=s_raw[:, cols].rearrange("p (m t) -> p t m", t=T),
-            )
+        def permute_scales():
+            nc.vector.tensor_copy(out=s_packed[:].rearrange("p (t m) -> p t m", t=T), in_=s_raw[:].rearrange("p (m t) -> p t m", t=T))
 
         def wide_tile(j0, count):
             wide = keep.tile([P, count, X], BF16, name="xv%d" % j0, align_bytes=64)
@@ -151,11 +146,6 @@ def tile_spn_w4_kernel(tc, x_bytes, x_scale, w0_words, w0_scales, w1_words, w1_s
             wide, codes = wide_tile(j0, count)
             halves_apart(j0, count, wide)
             nc.scalar.copy(out=wide[:].rearrange("p j (a m e) -> p j a m e", a=2, e=2), in_=codes.rearrange("p j (m a e) -> p j a m e", a=2, e=2))
-
-        def vector_cast(j):
-            wide, codes = wide_tile(j, 1)
-            halves_apart(j, 1, wide)
-            nc.vector.tensor_copy(out=wide[:, 0, :].rearrange("p (a m e) -> p m a e", a=2, e=2), in_=codes[:, 0, :].rearrange("p (m a e) -> p m a e", a=2, e=2))
 
         def scalar_first_cast(j):
             wide, codes = wide_tile(j, 1)
@@ -198,12 +188,11 @@ def tile_spn_w4_kernel(tc, x_bytes, x_scale, w0_words, w0_scales, w1_words, w1_s
 
         def plane(c, g, t, lo, z):
             m0 = PASS * g + P * t
-            s0 = PASS * (g % 2) + P * t
             cols = slice(lo, lo + z.shape[1])
             nc.tensor.matmul_mx(
                 out=z,
                 lhsT=w0_perm[:, 2 * m0 : 2 * (m0 + P)].bitcast(FP4X4),
-                lhsT_scale=(s_lo, s_hi)[g // 2][:, s0 : s0 + P],
+                lhsT_scale=s_perm[:, g, P * t : P * (t + 1)],
                 rhs=x_codes[c][:, cols].bitcast(FP8X4),
                 rhs_scale=x_scales[c][:, cols],
                 start=True,
@@ -363,6 +352,7 @@ def tile_spn_w4_kernel(tc, x_bytes, x_scale, w0_words, w0_scales, w1_words, w1_s
             gates[c, 1] = [("xq", c + 1, 0)] if c < last else [("q", c, 0, 0)]
 
         step("scalar", ("cast", 0), [("x", 0)], scalar_first_cast, 0)
+        s_cast(1, 1)
         s_cast(2, 2)
         s_cast(4, 2)
         s_cast(6, 2)
@@ -433,13 +423,12 @@ def tile_spn_w4_kernel(tc, x_bytes, x_scale, w0_words, w0_scales, w1_words, w1_s
         def v_relu(c, g=G - 1, lo=0):
             step("vector", ("relu", c, g), [], vector_relu, c, g, lo)
 
-        step("vector", ("cast", 1), [("x", 1)], vector_cast, 1)
+        step("vector", "scales", ["s_raw"], permute_scales)
         step("vector", ("words", 0), [("w0", 0)], permute_words, w0_lo[:, : 2 * PASS], 0, 1, nc.vector.tensor_copy)
         v_x(0, 1)
         v_x(1, 1)
-        step("vector", ("scales", 0), ["s_raw"], permute_scales, 0)
-        v_xq(0, 0, PAIR)
-        step("vector", ("scales", 1), [], permute_scales, 1)
+        v_xq(0, 0, P)
+        v_xq(0, P, PAIR)
         v_x(2, 2)
         step("vector", ("words", 2), [("w0", 2)], permute_words, w0_hi[:], 2, G, nc.vector.tensor_copy)
         v_xq(0, PAIR, CHUNK)
@@ -486,9 +475,8 @@ def tile_spn_w4_kernel(tc, x_bytes, x_scale, w0_words, w0_scales, w1_words, w1_s
         v_q(last, 3, PAIR, CHUNK)
         v_q(last, 1, PAIR, CHUNK)
         v_q(last, 2, 2 * P, 3 * P)
-        v_store(last, 0)
         v_q(last, 2, 3 * P, CHUNK)
-        for j in range(1, TILES):
+        for j in range(TILES):
             v_store(last, j)
 
         opened = []
@@ -507,7 +495,7 @@ def tile_spn_w4_kernel(tc, x_bytes, x_scale, w0_words, w0_scales, w1_words, w1_s
             return [k for k, n, f, a in lists["vector"] if k[: len(key)] == key and a[-2] < hi and a[-1] > lo]
 
         def weights_of(g):
-            return [("words", min(g, 2)), ("scales", g) if g < 2 else "s_hi"]
+            return [("words", min(g, 2)), "s_perm"]
 
         def t_x(j0, count):
             casts = [("cast", j) for j in (j0, j0 + count - 1) if j < 2 or j % 2 == 0]

from contextlib import ExitStack

import concourse.mybir as mybir
from concourse.masks import make_identity

F32 = mybir.dt.float32
BF16 = mybir.dt.bfloat16
U32 = mybir.dt.uint32
I32 = mybir.dt.int32
U16 = mybir.dt.uint16
U8 = mybir.dt.uint8
FP8 = mybir.dt.float8_e4m3fn
FP8X4 = mybir.dt.float8_e4m3fn_x4
FP4X4 = mybir.dt.float4_e2m1fn_x4
RELU = mybir.ActivationFunctionType.Relu
COPY = mybir.ActivationFunctionType.Copy
MULT = mybir.AluOpType.mult
ADD = mybir.AluOpType.add
MAX = mybir.AluOpType.max

P = 128
B, X, N, OS = 2048, 512, 2304, 256
H = N - OS
PASS = 512
G = H // PASS
T = 4
FLOPS = 2 * B * X * N + 2 * B * H * OS

TILES = 4
CHUNK = TILES * P
N_CHUNKS = B // CHUNK
PAIR = 2 * P
PLANE_BANKS = 4
SIDE_BANKS = 4
PLANE_PAD = 16
POOL_HEAD = 448
POOL_TAIL = 64
VECTOR_HEAD = 64


def tile_spn_w4_kernel(tc, x_bytes, x_scale, w0_words, w0_scales, w1_words, w1_scales, biases, out):
    nc = tc.nc
    last = N_CHUNKS - 1
    x_view = x_bytes.rearrange("(p j) k -> p j k", j=B // P)
    out_view = out.rearrange("(p j) n -> p j n", j=B // P)

    with ExitStack() as ctx:
        keep = ctx.enter_context(tc.tile_pool(name="keep", bufs=1))
        psum = ctx.enter_context(tc.psum_pool(name="psum", bufs=PLANE_BANKS))
        ctx.enter_context(tc.manual_schedule())

        ident = keep.tile([P, P], F32, name="ident")
        w0_lo = keep.tile([P, 4 * PASS], U8, name="w0_lo", align_bytes=64)
        w0_hi = keep.tile([P, 4 * PASS], U8, name="w0_hi", tag="gate0", align_bytes=64)
        w0_out = keep.tile([P, 2 * OS], U8, name="w0_out", align_bytes=64)
        w0_perm = keep.tile([P, 2 * H], U8, name="w0_perm", align_bytes=64)
        s_raw = keep.tile([P, PASS], U8, name="s_raw", align_bytes=64)
        s_packed = keep.tile([P, PASS], U8, name="s_packed", align_bytes=64)
        s_perm = keep.tile([P, G, PASS], U8, name="s_perm", align_bytes=64)
        w1 = keep.tile([P, G, 2 * OS], U8, name="w1", align_bytes=64)
        s_out = keep.tile([P, G + 1, OS], U8, name="s_out", align_bytes=64)
        bias_h = keep.tile([P, G, T], BF16, name="bias_h")
        bias_o = keep.tile([P, OS], BF16, name="bias_o")
        xs_col = keep.tile([P, T], F32, name="xs_col")

        nc.vector.memset(s_raw[:].bitcast(I32), 0)
        nc.vector.memset(s_perm[:].rearrange("p g n -> p (g n)").bitcast(I32), 0)
        nc.vector.memset(s_out[:].rearrange("p g n -> p (g n)").bitcast(I32), 0)
        make_identity(nc, ident[:])

        lists = {"sync": [], "tensor": [], "scalar": [], "vector": [], "pool": []}

        def step(engine, key, needs, call, *args):
            lists[engine].append((key, list(needs), call, args))

        x_raw, x_wide, x_woven, x_codes, x_scales = {}, {}, {}, {}, {}
        h_planes, h_woven, h_codes, h_scales, z_pairs, banks = {}, {}, {}, {}, {}, {}

        def load_x(j0, count):
            raw = keep.tile([P, count, X], U8, name="xbytes%d" % j0, align_bytes=64)
            for jj in range(count):
                x_raw[j0 + jj] = (raw, jj)
            nc.sync.dma_start(out=raw[:], in_=x_view[:, j0 : j0 + count, :])

        def load(dst, src):
            nc.sync.dma_start(out=dst, in_=src)

        def w0_cols(n0, n1):
            return w0_words[0, :, 2 * n0 : 2 * n1]

        def load_hidden_scales():
            rows = w0_scales[0, :, 0:H].bitcast(I32).rearrange("r (g n) -> r g n", g=G)
            nc.sync.dma_start(out=s_raw[0 : 16 * G, :].bitcast(I32), in_=rows)

        def spread_scales():
            for q in range(4):
                nc.sync.dma_start(out=s_perm[32 * q : 32 * q + 4].bitcast(I32), in_=s_packed[16 * q : 16 * q + 16, :].bitcast(I32))

        def load_out_scales():
            for r in range(4):
                nc.sync.dma_start(out=s_out[r:P:32, G, :].bitcast(I32), in_=w0_scales[0, r:16:4, H:N].bitcast(I32))
            for r in range(4):
                nc.sync.dma_start(out=s_out[r:P:32, 0:G, :].bitcast(I32), in_=w1_scales[:, r:16:4, :].rearrange("g q n -> q g n").bitcast(I32))

        x_loads = ((0, 1), (1, 1), (2, 2), (4, 2), (6, 2), (8, 2), (10, 6))
        x_load_of = {j0 + jj: ("x", j0) for j0, count in x_loads for jj in range(count)}
        step("sync", ("x", 0), [], load_x, 0, 1)
        step("sync", ("x", 1), [], load_x, 1, 1)
        step("sync", "s_raw", [], load_hidden_scales)
        step("sync", ("x", 2), [], load_x, 2, 2)
        step("sync", ("w0", 0), [], load, w0_lo[:, : 2 * PASS], w0_cols(0, PASS))
        step("sync", "xs", [], load, xs_col[:], x_scale.rearrange("o (p t) -> p (o t)", t=T))
        step("sync", ("x", 4), [], load_x, 4, 2)
        step("sync", ("x", 6), [], load_x, 6, 2)
        step("sync", ("w0", 1), [], load, w0_lo[:, 2 * PASS :], w0_cols(PASS, 2 * PASS))
        step("sync", "bias_h", [], load, bias_h[:], biases[0:H].rearrange("(g p t) -> p g t", g=G, p=P, t=T))
        step("sync", "s_perm", ["scales"], spread_scales)
        step("sync", ("x", 8), [], load_x, 8, 2)
        step("sync", ("w0", 2), [], load, w0_hi[:], w0_cols(2 * PASS, H))
        step("sync", ("x", 10), [], load_x, 10, 6)
        step("sync", "w0_out", [], load, w0_out[:], w0_cols(H, N))
        step("sync", "w1", [], load, w1[:], w1_words.rearrange("g p n -> p g n"))
        step("sync", "s_out", [], load_out_scales)
        step("sync", "bias_o", [], load, bias_o[:], biases[H:N].partition_broadcast(P))

        def permute_words(raw, g0, g1, copy):
            copy(
                out=w0_perm[:, 2 * PASS * g0 : 2 * PASS * g1].bitcast(U16).rearrange("p (g t m) -> p g t m", t=T, m=P),
                in_=raw.bitcast(U16).rearrange("p (g m t) -> p g t m", t=T, m=P),
            )

        def permute_scales():
            nc.vector.tensor_copy(out=s_packed[:].rearrange("p (t m) -> p t m", t=T), in_=s_raw[:].rearrange("p (m t) -> p t m", t=T))

        def wide_tile(j0, count):
            wide = keep.tile([P, count, X], BF16, name="xv%d" % j0, align_bytes=64)
            raw, first = x_raw[j0]
            return wide, raw[:, first : first + count, :].bitcast(FP8)

        def halves_apart(j0, count, wide):
            for jj in range(count):
                words = wide[:, jj, :].bitcast(F32)
                x_wide[j0 + jj] = (words[:, :P], words[:, P:])

        def scalar_cast(j0, count):
            wide, codes = wide_tile(j0, count)
            halves_apart(j0, count, wide)
            nc.scalar.copy(out=wide[:].rearrange("p j (a m e) -> p j a m e", a=2, e=2), in_=codes.rearrange("p j (m a e) -> p j a m e", a=2, e=2))

        def scalar_first_cast(j):
            wide, codes = wide_tile(j, 1)
            halves_apart(j, 1, wide)
            halves = wide[:, 0, :].rearrange("p (a m e) -> p a m e", a=2, e=2)
            pairs = codes[:, 0, :].rearrange("p (m a e) -> p a m e", a=2, e=2)
            nc.scalar.activation(out=halves[:, 0, 0, :], in_=pairs[:, 0, 0, :], func=COPY)
            nc.scalar.copy(out=halves[:, 0, 1:, :], in_=pairs[:, 0, 1:, :])
            nc.scalar.copy(out=halves[:, 1], in_=pairs[:, 1])

        side_tag = {}

        def side_bank(job, shape, name):
            banks[job] = psum.tile(shape, F32, name=name, tag=side_tag[job], bufs=1)
            return banks[job]

        def x_transpose(j0, count):
            bank = side_bank(("xt", j0), [P, 2, count, P], "xt")
            for jj in range(count):
                for a in range(2):
                    nc.tensor.transpose(bank[:, a, jj, :], x_wide[j0 + jj][a], ident[:])

        def x_scale_out(j0, count):
            c, at = divmod(j0, TILES)
            if c not in x_woven:
                x_woven[c] = keep.tile([P, T * CHUNK], BF16, name="xg", tag="mid%d" % (c - 1), align_bytes=64)
            values = banks["xt", j0][:].rearrange("p a j r -> p (a j r)").bitcast(BF16)
            nc.vector.tensor_tensor(
                out=x_woven[c][:, T * P * at : T * P * (at + count)].rearrange("p (r a e) -> p r a e", a=2, e=2),
                in0=values.rearrange("p (a r e) -> p r a e", a=2, e=2),
                in1=xs_col[:].rearrange("p (o a e) -> p o a e", o=1, a=2).to_broadcast([P, count * P, 2, 2]),
                op=MULT,
            )

        def x_quantize(c, lo, hi):
            if lo == 0:
                x_codes[c] = keep.tile([P, CHUNK], U32, name="xq%d" % c, align_bytes=64)
                x_scales[c] = keep.tile([P, CHUNK], U8, name="xqs%d" % c, align_bytes=64)
            nc.vector.quantize_mx(out=x_codes[c][:, lo:hi].bitcast(FP8X4), scales=x_scales[c][:, lo:hi], in_=x_woven[c][:, T * lo : T * hi])

        def plane(c, g, t, lo, z):
            m0 = PASS * g + P * t
            cols = slice(lo, lo + z.shape[1])
            nc.tensor.matmul_mx(
                out=z,
                lhsT=w0_perm[:, 2 * m0 : 2 * (m0 + P)].bitcast(FP4X4),
                lhsT_scale=s_perm[:, g, P * t : P * (t + 1)],
                rhs=x_codes[c][:, cols].bitcast(FP8X4),
                rhs_scale=x_scales[c][:, cols],
                start=True,
                stop=True,
            )

        def planes_view(c, u):
            if (c, u) not in h_planes:
                h_planes[c, u] = keep.tile([P, T, CHUNK + PLANE_PAD], BF16, name="hp%d_%d" % (c, u), align_bytes=64)
            return h_planes[c, u]

        def ring_fill(job):
            c, g, t0, count, lo, width = job
            banks[job] = psum.tile([P, count, width], F32, name="z", bufs=PLANE_BANKS)
            for i in range(count):
                plane(c, g, t0 + i, lo, banks[job][:, i, :])

        def ring_out(job):
            c, g, t0, count, lo, width = job
            u, at = (lo // PAIR, PAIR * g) if c == 0 and g < 2 else (g, lo)
            for i in range(count):
                t = t0 + i
                nc.scalar.activation(out=planes_view(c, u)[:, t, at : at + width], in_=banks[job][:, i, :], func=RELU, bias=bias_h[:, g, t : t + 1])

        def pair_fill(c, g, i):
            pair, a = divmod(i, 2)
            bank = side_bank(("zv", c, g, i), [P, 2, PAIR], "zv")
            for e in range(2):
                plane(c, g, 2 * a + e, PAIR * pair, bank[:, e, :])

        def pair_out(c, g, i):
            pair, a = divmod(i, 2)
            if (c, g) not in z_pairs:
                z_pairs[c, g] = keep.tile([P, 2, 2 * CHUNK + PLANE_PAD], BF16, name="zg%d_%d" % (c, g), align_bytes=64)
            nc.vector.tensor_tensor(
                out=z_pairs[c, g][:, a, 2 * PAIR * pair : 2 * PAIR * (pair + 1)].rearrange("p (n e) -> p n e", e=2),
                in0=banks["zv", c, g, i][:].rearrange("p e n -> p n e"),
                in1=bias_h[:, g, 2 * a : 2 * a + 2].unsqueeze(1).to_broadcast([P, PAIR, 2]),
                op=ADD,
            )

        def woven_tag(c, u):
            if u == 0:
                return "gate%d" % c
            if u == G - 1:
                return "gate%d" % (c + 1)
            if u == 1:
                return "mid%d" % c if c < last else "gate%d" % c
            return "third%d" % c

        def woven_view(c, u):
            if (c, u) not in h_woven:
                h_woven[c, u] = keep.tile([P, T * CHUNK], BF16, name="hg", tag=woven_tag(c, u), align_bytes=64)
            return h_woven[c, u]

        def vector_relu(c, g, lo):
            nc.vector.tensor_scalar(
                out=woven_view(c, g)[:, T * lo :].rearrange("p (n a e) -> p n a e", a=2, e=2),
                in0=z_pairs[c, g][:, :, 2 * lo : 2 * CHUNK].rearrange("p a (n e) -> p n a e", e=2),
                scalar1=0.0,
                scalar2=None,
                op0=MAX,
            )

        def weave(copy, c, u, lo, hi):
            copy(
                out=woven_view(c, u)[:, T * lo : T * hi].rearrange("p (c i t) -> p c t i", t=T, i=4),
                in_=planes_view(c, u)[:, :, lo:hi].rearrange("p t (c i) -> p c t i", i=4),
            )

        def pool_weave(c, u, lo, hi):
            nc.gpsimd.tensor_scalar(
                out=woven_view(c, u)[:, T * lo : T * hi].rearrange("p (c i t) -> p c t i", t=T, i=4),
                in0=planes_view(c, u)[:, :, lo:hi].rearrange("p t (c i) -> p c t i", i=4),
                scalar1=1.0,
                scalar2=0.0,
                op0=MULT,
                op1=ADD,
            )

        def h_quantize(c, u, lo, hi):
            if (c, u) not in h_codes:
                h_codes[c, u] = keep.tile([P, CHUNK], U32, name="hq%d_%d" % (c, u), align_bytes=64)
                h_scales[c, u] = keep.tile([P, CHUNK], U8, name="hqs%d_%d" % (c, u), align_bytes=64)
            nc.vector.quantize_mx(out=h_codes[c, u][:, lo:hi].bitcast(FP8X4), scales=h_scales[c, u][:, lo:hi], in_=woven_view(c, u)[:, T * lo : T * hi])

        def sum_job(c, j):
            return (("o", c, j), 1, 0) if c == last else (("o", c, j - j % 2), 2, j % 2)

        def unit_place(c, g, j):
            return (j // 2, 2 * g + j % 2) if c == 0 and g < 2 else (g, j)

        def out_pass(c, j, g, closes):
            job, count, place = sum_job(c, j)
            opens = g == G and place == 0
            if opens:
                side_bank(job, [P, count, OS], "o")
            if g == G:
                at, codes, scales, w = j, x_codes[c], x_scales[c], w0_out[:]
            else:
                u, at = unit_place(c, g, j)
                codes, scales, w = h_codes[c, u], h_scales[c, u], w1[:, g, :]
            cols = slice(at * P, (at + 1) * P)
            nc.tensor.matmul_mx(
                out=banks[job][:, place, :],
                lhsT=codes[:, cols].bitcast(FP8X4),
                lhsT_scale=scales[:, cols],
                rhs=w.bitcast(FP4X4),
                rhs_scale=s_out[:, g, :],
                start=opens,
                stop=closes,
            )

        def store(c, j0):
            job, count, place = sum_job(c, j0)
            res = keep.tile([P, count, OS], F32, name="res%d_%d" % (c, j0))
            nc.vector.tensor_tensor(out=res[:], in0=banks[job][:], in1=bias_o[:].unsqueeze(1).to_broadcast([P, count, OS]), op=ADD)
            nc.sync.dma_start(out=out_view[:, TILES * c + j0 : TILES * c + j0 + count, :], in_=res[:])

        ring = []

        def s_cast(j0, count):
            step("scalar", ("cast", j0), [x_load_of[j0]], scalar_cast, j0, count)

        def s_planes(c, g, t0, count, lo, width):
            job = (c, g, t0, count, lo, width)
            ring.append(job)
            step("scalar", ("out", job), [("fill", job), "bias_h"], ring_out, job)

        def s_unit(c, g, planes=T):
            for t in range(planes):
                s_planes(c, g, t, 1, 0, CHUNK)

        def planes_done(c, u, lo):
            if c == 0 and u < 2:
                return ("out", (0, lo // PAIR, 2, 2, PAIR * u, PAIR))
            if c == 0:
                return ("out", (0, u, 2, 2, 0, PAIR))
            if (c, u) == (last - 1, 2):
                return ("out", (c, u, T - 1, 1, lo - lo % PAIR, PAIR))
            return ("out", (c, u, T - 1, 1, 0, CHUNK))

        gates = {}

        def weave_step(engine, c, u, lo, hi):
            needs = [planes_done(c, u, lo), planes_done(c, u, hi - 1)] + gates.get((c, u), [])
            if engine == "pool":
                step(engine, ("weave", c, u, lo), needs, pool_weave, c, u, lo, hi)
            else:
                copy = nc.scalar.copy if engine == "scalar" else nc.vector.tensor_copy
                step(engine, ("weave", c, u, lo), needs, weave, copy, c, u, lo, hi)

        gates[0, 0] = [("words", 2)]
        for c in range(N_CHUNKS):
            if c > 0:
                gates[c, 0] = [("q", c - 1, G - 1, 0)]
            gates[c, 1] = [("xq", c + 1, 0)] if c < last else [("q", c, 0, 0)]

        step("scalar", ("cast", 0), [("x", 0)], scalar_first_cast, 0)
        s_cast(1, 1)
        s_cast(2, 2)
        s_cast(4, 2)
        s_cast(6, 2)
        step("scalar", ("words", 1), [("w0", 1)], permute_words, w0_lo[:, 2 * PASS :], 1, 2, nc.scalar.copy)
        s_cast(8, 2)
        s_planes(0, 0, 0, 1, 0, PAIR)
        s_planes(0, 0, 1, 1, 0, PAIR)
        s_planes(0, 0, 2, 2, 0, PAIR)
        for t0 in (0, 2):
            s_planes(0, 1, t0, 2, 0, PAIR)
        for g in range(2):
            for t0 in (0, 2):
                s_planes(0, g, t0, 2, PAIR, PAIR)
        for t0 in (0, 2):
            s_planes(0, 2, t0, 2, 0, PAIR)
        s_cast(10, 2)
        s_cast(12, 2)
        weave_step("scalar", 0, 2, VECTOR_HEAD, PAIR)
        for c in range(1, N_CHUNKS):
            s_unit(c, 0)
            s_unit(c, 1)
            if c == last - 1:
                s_unit(c, 2, T - 1)
                for lo in (0, PAIR):
                    s_planes(c, 2, T - 1, 1, lo, PAIR)
                for lo in (0, PAIR):
                    weave_step("scalar", c, 2, lo, lo + PAIR)
            else:
                s_unit(c, 2)
            if c == 1:
                s_cast(14, 2)
                weave_step("scalar", c, 2, 0, CHUNK)
        weave_step("scalar", last, 1, POOL_TAIL, PAIR)
        weave_step("scalar", last, 1, PAIR, CHUNK)
        for j in (2, 3):
            weave_step("scalar", last, 2, P * j, P * (j + 1))

        weave_step("pool", 0, 0, 0, PAIR)
        weave_step("pool", 0, 0, PAIR, CHUNK)
        weave_step("pool", 0, 1, 0, POOL_HEAD)
        for c in range(1, N_CHUNKS):
            weave_step("pool", c, 0, 0, CHUNK)
            weave_step("pool", c, 1, 0, CHUNK if c < last else POOL_TAIL)

        reads = []

        def v_read(job, needs, call, *args):
            reads.append(job)
            step("vector", ("out", job), [("fill", job)] + needs, call, *args)

        def v_x(j0, count):
            v_read(("xt", j0), ["xs"], x_scale_out, j0, count)

        def v_pair(c, i, g=G - 1):
            v_read(("zv", c, g, i), ["bias_h"], pair_out, c, g, i)

        def v_store(c, j0):
            v_read(("o", c, j0), ["bias_o"], store, c, j0)

        def v_xq(c, lo, hi):
            needs = [key for key, n, f, a in lists["vector"] if key[0] == "out" and key[1][0] == "xt"]
            step("vector", ("xq", c, lo), needs, x_quantize, c, lo, hi)

        def v_q(c, u, lo=0, hi=CHUNK):
            needs = [key for engine in ("scalar", "pool") for key, n, f, a in lists[engine] if key[:3] == ("weave", c, u) and a[-2] < hi and a[-1] > lo]
            step("vector", ("q", c, u, lo), needs, h_quantize, c, u, lo, hi)

        def v_relu(c, g=G - 1, lo=0):
            step("vector", ("relu", c, g), [], vector_relu, c, g, lo)

        step("vector", "scales", ["s_raw"], permute_scales)
        step("vector", ("words", 0), [("w0", 0)], permute_words, w0_lo[:, : 2 * PASS], 0, 1, nc.vector.tensor_copy)
        v_x(0, 1)
        v_x(1, 1)
        v_xq(0, 0, P)
        v_xq(0, P, PAIR)
        v_x(2, 2)
        step("vector", ("words", 2), [("w0", 2)], permute_words, w0_hi[:], 2, G, nc.vector.tensor_copy)
        v_xq(0, PAIR, CHUNK)
        v_x(4, 2)
        v_x(6, 2)
        v_pair(0, 0)
        v_pair(0, 1)
        v_xq(1, 0, CHUNK)
        v_q(0, 0)
        v_pair(0, 2)
        v_pair(0, 3)
        v_pair(0, 2, 2)
        v_pair(0, 3, 2)
        v_relu(0)
        weave_step("vector", 0, 1, POOL_HEAD, CHUNK)
        v_relu(0, 2, PAIR)
        weave_step("vector", 0, 2, 0, VECTOR_HEAD)
        for c in range(last):
            d = c + 1
            if c > 0:
                v_relu(c)
            for u in (1, 3, 2):
                v_q(c, u)
            if d < last:
                v_x(TILES * (d + 1), 2)
                v_x(TILES * (d + 1) + 2, 2)
                v_store(c, 0)
                v_xq(d + 1, 0, CHUNK)
                v_q(d, 0)
                for i in range(4):
                    v_pair(d, i)
                v_store(c, 2)
        v_pair(last, 0)
        v_pair(last, 1)
        v_store(last - 1, 0)
        v_pair(last, 2)
        v_pair(last, 3)
        v_q(last, 0)
        v_relu(last)
        v_store(last - 1, 2)
        weave_step("vector", last, 2, 0, PAIR)
        for u in (3, 1, 2):
            v_q(last, u, 0, PAIR)
        v_q(last, 3, PAIR, CHUNK)
        v_q(last, 1, PAIR, CHUNK)
        v_q(last, 2, 2 * P, 3 * P)
        v_q(last, 2, 3 * P, CHUNK)
        for j in range(TILES):
            v_store(last, j)

        opened = []
        filled = []

        def freed(job):
            n = len(opened)
            opened.append(job)
            if n < SIDE_BANKS:
                side_tag[job] = "side%d" % n
                return []
            side_tag[job] = side_tag[reads[n - SIDE_BANKS]]
            return [("out", reads[n - SIDE_BANKS])]

        def codes_of(key, lo, hi):
            return [k for k, n, f, a in lists["vector"] if k[: len(key)] == key and a[-2] < hi and a[-1] > lo]

        def weights_of(g):
            return [("words", min(g, 2)), "s_perm"]

        def t_x(j0, count):
            casts = [("cast", j) for j in (j0, j0 + count - 1) if j < 2 or j % 2 == 0]
            step("tensor", ("fill", ("xt", j0)), casts + freed(("xt", j0)), x_transpose, j0, count)

        def t_planes(count):
            for i in range(count):
                n = len(filled)
                job = ring[n]
                filled.append(job)
                c, g, t0, planes, lo, width = job
                needs = codes_of(("xq", c), lo, lo + width) + weights_of(g)
                if n >= PLANE_BANKS:
                    needs.append(("out", ring[n - PLANE_BANKS]))
                step("tensor", ("fill", job), needs, ring_fill, job)

        def t_pair(c, i, g=G - 1):
            lo = PAIR * (i // 2)
            needs = codes_of(("xq", c), lo, lo + PAIR) + weights_of(g) + freed(("zv", c, g, i))
            step("tensor", ("fill", ("zv", c, g, i)), needs, pair_fill, c, g, i)

        def t_pass(c, j, g, closing=False):
            job, count, place = sum_job(c, j)
            if g == G:
                needs = ["w0_out", "s_out"] + (freed(job) if place == 0 else [])
            else:
                u, at = unit_place(c, g, j)
                needs = ["w1"] + codes_of(("q", c, u), P * at, P * (at + 1))
            closes = closing and place == count - 1
            step("tensor", ("fill", job) if closes else ("pass", c, j, g), needs, out_pass, c, j, g, closes)

        def t_passes(c, pair, g, closing=False):
            for j in (2 * pair, 2 * pair + 1):
                t_pass(c, j, g, closing)

        t_x(0, 1)
        t_x(1, 1)
        t_x(2, 2)
        t_x(4, 2)
        t_planes(5)
        t_x(6, 2)
        t_planes(1)
        t_pair(0, 0)
        t_planes(1)
        t_pair(0, 1)
        t_planes(2)
        t_pair(0, 2)
        t_planes(1)
        t_pair(0, 3)
        t_planes(1)
        t_pair(0, 2, 2)
        t_pair(0, 3, 2)
        for c in range(last):
            d = c + 1
            t_planes(2)
            if c > 0:
                t_pair(c, 3)
            t_planes(2)
            if d < last:
                t_x(TILES * (d + 1), 2)
                t_x(TILES * (d + 1) + 2, 2)
                t_passes(c, 0, G)
                t_passes(c, 0, 0)
                t_pair(d, 0)
                t_planes(T)
                t_passes(c, 0, 1)
                t_passes(c, 0, 3)
                t_passes(c, 0, 2, True)
                t_planes(3)
                t_passes(c, 1, G)
                t_passes(c, 1, 0)
                t_planes(d)
                t_passes(c, 1, 1)
                t_pair(d, 1)
                t_pair(d, 2)
                t_passes(c, 1, 3)
                t_passes(c, 1, 2, True)
        c = last - 1
        t_pair(last, 0)
        t_pair(last, 1)
        t_passes(c, 0, G)
        t_passes(c, 0, 0)
        t_pair(last, 2)
        t_planes(2)
        t_passes(c, 0, 1)
        t_planes(1)
        t_passes(c, 0, 3)
        t_planes(1)
        t_passes(c, 0, 2, True)
        t_planes(1)
        t_pair(last, 3)
        t_planes(1)
        t_passes(c, 1, G)
        t_planes(1)
        t_passes(c, 1, 0)
        t_planes(1)
        t_passes(c, 1, 1)
        t_passes(c, 1, 3)
        t_passes(c, 1, 2, True)
        for j in range(3):
            t_pass(last, j, G)
        for j in range(3):
            t_pass(last, j, 0)
        t_pass(last, 3, G)
        t_pass(last, 3, 0)
        for g in (3, 1):
            t_passes(last, 0, g)
        t_passes(last, 0, 2, True)
        t_passes(last, 1, 3)
        t_passes(last, 1, 1)
        t_passes(last, 1, 2, True)

        done = set()
        at = {engine: 0 for engine in lists}
        for sweep in range(sum(len(steps) for steps in lists.values())):
            for engine, steps in lists.items():
                for key, needs, call, args in steps[at[engine] :]:
                    if not all(need in done for need in needs):
                        break
                    call(*args)
                    done.add(key)
                    at[engine] = at[engine] + 1
        assert all(at[engine] == len(steps) for engine, steps in lists.items())
